import numpy as np
import ml_dtypes


def mxq(x, axis, fmt="e4m3"):
    dtype, down = {"e4m3": (ml_dtypes.float8_e4m3fn, 7), "e5m2": (ml_dtypes.float8_e5m2, 14)}[fmt]
    v = np.moveaxis(np.asarray(x, np.float32).astype(ml_dtypes.bfloat16).astype(np.float64), axis, -1)
    blocks = v.reshape(v.shape[:-1] + (-1, 32))
    amax = np.abs(blocks).max(-1, keepdims=True)
    byte = np.maximum(np.where(amax > 0, np.frexp(amax)[1] - 1 + 127, 0) - down, 1)
    scale = np.exp2(byte - 127.0)
    codes = (blocks / scale).astype(np.float32).astype(dtype).astype(np.float64)
    return np.moveaxis((codes * scale).reshape(v.shape), -1, axis)


WIDE = False


def mx_kscale(k):
    if not WIDE:
        return np.ones(k)
    levels = np.array([18, -18])
    if k % 512:
        return np.exp2(np.random.permutation(np.resize(levels, k // 32))).repeat(32)
    a = np.empty((k // 512, 16))
    for p in range(k // 512):
        a[p, :8] = np.random.permutation(np.resize(levels, 8))
        for g in range(8):
            far = levels[np.abs(levels - a[p, g]) >= 10]
            a[p, g + 8] = far[np.random.randint(len(far))]
    return np.exp2(a.ravel()).repeat(32)


BF16 = ml_dtypes.bfloat16


def bf(x):
    return np.asarray(x, np.float32).astype(BF16)


def f64(x):
    return np.asarray(x).astype(np.float64)


J, N, X, H, Y = 2, 1024, 1024, 1024, 512
B1 = 2.0 / np.sqrt(X)
B2 = 2.0 / np.sqrt(H)
GAP = 2.0 ** -11


def uni(*sh):
    return np.random.random_sample(sh)


def sample(mu, e, sig):
    return f64(mu) + f64(e) * f64(sig)


def setup_inputs():
    s = mx_kscale(N)[:, None]
    u = mx_kscale(Y)
    v = mx_kscale(H)
    x0 = bf(np.random.standard_normal((N, X)))
    mu_W1 = bf(B1 * (uni(X, H) - 0.5))
    mu_b1 = bf(0.6 * (uni(1, H) - 0.5))
    mu_W2 = bf(B2 * (uni(H, Y) - 0.5))
    mu_b2 = bf(0.6 * (uni(1, Y) - 0.5))
    sig_W1 = bf(B1 * uni(X, H))
    sig_b1 = bf(0.4 * uni(1, H))
    sig_W2 = bf(B2 * uni(H, Y))
    sig_b2 = bf(0.4 * uni(1, Y))
    e_W1 = bf(np.random.standard_normal((J, X, H)))
    e_b1 = bf(np.random.standard_normal((J, 1, H)))
    e_W2 = bf(np.random.standard_normal((J, H, Y)))
    e_b2 = bf(np.random.standard_normal((J, 1, Y)))
    W1 = sample(mu_W1, e_W1, sig_W1)
    b1 = sample(mu_b1, e_b1, sig_b1)
    xf = f64(x0)
    z1 = xf @ W1 + b1
    while True:
        bad = np.nonzero((np.abs(np.abs(z1) - 1.0) < GAP).any(axis=(0, 2)))[0]
        if bad.size == 0:
            break
        xf[bad] = f64(bf(np.random.standard_normal((bad.size, X))))
        z1[:, bad] = xf[bad] @ W1 + b1
    g = 2.0 * np.random.standard_normal((J, N, Y)) * np.exp2(np.random.randint(-6, 1, (J, N, 1)))
    return {
        "x": bf(xf * s),
        "mu_W1": bf(f64(mu_W1) / v),
        "mu_b1": mu_b1,
        "mu_W2": bf(f64(mu_W2) * v[:, None] / u),
        "mu_b2": mu_b2,
        "sig_W1": bf(f64(sig_W1) / v),
        "sig_b1": sig_b1,
        "sig_W2": bf(f64(sig_W2) * v[:, None] / u),
        "sig_b2": sig_b2,
        "e_W1": e_W1,
        "e_b1": e_b1,
        "e_W2": e_W2,
        "e_b2": e_b2,
        "z1": np.asarray(z1, np.float32),
        "grad_out": bf(g / s * u),
    }


def reference(x, mu_W1, mu_b1, mu_W2, mu_b2, sig_W1, sig_b1, sig_W2, sig_b2, e_W1, e_b1, e_W2, e_b2, z1, grad_out):
    W1 = sample(mu_W1, e_W1, sig_W1)
    W2 = sample(mu_W2, e_W2, sig_W2)
    gq = mxq(f64(grad_out), 2, "e5m2")
    w2q = mxq(W2, 2, "e4m3")
    dh = gq @ w2q.transpose(0, 2, 1)
    dz1 = dh * (np.abs(f64(z1)) < 1.0)
    w1q = mxq(W1, 2, "e4m3")
    dx = (mxq(dz1, 2, "e5m2") @ w1q.transpose(0, 2, 1)).sum(axis=0)
    xq = mxq(f64(x), 0, "e4m3")
    dW1 = xq.T @ mxq(dz1, 1, "e5m2")
    dsig_W1 = (f64(e_W1) * dW1).sum(axis=0)
    return dx, dsig_W1

@@ -1,0 +1,364 @@
+from contextlib import ExitStack
+
+import concourse.mybir as mybir
+from concourse.masks import make_identity
+
+J, N, X, H, Y = 2, 1024, 1024, 1024, 512
+
+F32 = mybir.dt.float32
+BF16 = mybir.dt.bfloat16
+U32 = mybir.dt.uint32
+U8 = mybir.dt.uint8
+E4M3 = mybir.dt.float8_e4m3fn_x4
+E5M2 = mybir.dt.float8_e5m2_x4
+ALU = mybir.AluOpType
+ACT = mybir.ActivationFunctionType
+
+FLOPS = J * (2 * N * Y * H + 2 * N * H * X + 2 * N * H * X)
+BYTES = 2 * (N * X + 2 * X * H + J * X * H + 2 * H * Y + J * H * Y + J * N * Y) + 4 * (J * N * H + N * X + X * H)
+
+P = 128
+T = 4
+
+
+def tile_gaussian_nn_htanh_v_kernel(
+    tc, x, mu_W1, mu_b1, mu_W2, mu_b2, sig_W1, sig_b1, sig_W2, sig_b2, e_W1, e_b1, e_W2, e_b2, z1, grad_out, out_0, out_1
+):
+    nc = tc.nc
+
+    with ExitStack() as ctx:
+        const = ctx.enter_context(tc.tile_pool(name="const", bufs=1))
+        raw = ctx.enter_context(tc.tile_pool(name="raw", bufs=2))
+        work = ctx.enter_context(tc.tile_pool(name="work", bufs=2))
+        codes = ctx.enter_context(tc.tile_pool(name="codes", bufs=1))
+        psum = ctx.enter_context(tc.psum_pool(name="psum", bufs=4))
+
+        ident_f = const.tile([P, P], F32, name="ident_f", tag="ident_f")
+        make_identity(nc, ident_f[:])
+        ident_b = const.tile([P, P], BF16, name="ident_b", tag="ident_b")
+        nc.vector.tensor_copy(out=ident_b[:], in_=ident_f[:])
+
+        def copy_to(engine, out, in_):
+            if engine == "s":
+                nc.scalar.copy(out=out, in_=in_)
+            else:
+                nc.vector.tensor_copy(out=out, in_=in_)
+
+        def code_tile(name, width, tag, bufs):
+            c = codes.tile([P, width], U32, name=name, tag=tag, bufs=bufs, align_bytes=64)
+            s = codes.tile([P, width], U8, name=name + "_s", tag=tag + "_s", bufs=bufs, align_bytes=64)
+            return c, s
+
+        def quantize(dst, c0, c1, fmt, src):
+            nc.vector.quantize_mx(out=dst[0][:, c0:c1].bitcast(fmt), scales=dst[1][:, c0:c1], in_=src)
+
+        def grp_tile(name):
+            return work.tile([P, 512, T], BF16, name=name, tag="grp", bufs=6, align_bytes=64)
+
+        def load_w2_const(q):
+            v = sig_W2.rearrange("(q b m) y -> q m b y", q=2, b=4)
+            sg = raw.tile([P, 4, Y], BF16, name="sg2", tag="w2s", bufs=4)
+            nc.sync.dma_start(out=sg[:], in_=v[q])
+            v = mu_W2.rearrange("(q b m) y -> q m b y", q=2, b=4)
+            mu = raw.tile([P, 4, Y], BF16, name="mu2", tag="w2s", bufs=4)
+            nc.sync.dma_start(out=mu[:], in_=v[q])
+            return sg, mu
+
+        def load_e2(j, q):
+            v = e_W2[j].rearrange("(q b m) y -> q m b y", q=2, b=4)
+            e = raw.tile([P, 4, Y], BF16, name="e2", tag="in4", bufs=4)
+            nc.sync.dma_start(out=e[:], in_=v[q])
+            return e
+
+        def load_grad(j, g):
+            v = grad_out[j].rearrange("(g p t) y -> g p t y", g=2, t=T)
+            t = raw.tile([P, T, Y], BF16, name="gr", tag="in4", bufs=4)
+            nc.sync.dma_start(out=t[:], in_=v[g])
+            return t
+
+        def load_x(g, half):
+            v = x.rearrange("(g p t) w -> g p t w", g=2, t=T)
+            t = raw.tile([P, T, 512], BF16, name="xr", tag="in4", bufs=4)
+            nc.sync.dma_start(out=t[:], in_=v[g][:, :, 512 * half : 512 * half + 512])
+            return t
+
+        def load_z(j, g, t):
+            v = z1[j].rearrange("(g p t) h -> g t p h", g=2, t=T)
+            zt = raw.tile([P, H], F32, name="z", tag="z", bufs=4)
+            nc.sync.dma_start(out=zt[:], in_=v[g, t])
+            return zt
+
+        def load_w1(i):
+            rows = slice(P * i, P * i + P)
+            sg = raw.tile([P, H], BF16, name="sg1", tag="sg1", bufs=3)
+            nc.sync.dma_start(out=sg[:], in_=sig_W1[rows, :])
+            es = []
+            for j in range(J):
+                e = raw.tile([P, H], BF16, name="e1", tag="e1", bufs=16)
+                nc.sync.dma_start(out=e[:], in_=e_W1[j][rows, :])
+                es.append(e)
+            mu = raw.tile([P, H], BF16, name="mu1", tag="mu1", bufs=3)
+            nc.sync.dma_start(out=mu[:], in_=mu_W1[rows, :])
+            return sg, es, mu
+
+        def multiply(engine, e, sg):
+            prod = work.tile([P, 2, T, P], F32, name="prod", tag="prod", bufs=3)
+            eng = nc.gpsimd if engine == "g" else nc.vector
+            eng.tensor_tensor(
+                out=prod[:],
+                in0=e.rearrange("p b (w t) -> p b t w", t=T),
+                in1=sg.rearrange("p b (w t) -> p b t w", t=T),
+                op=ALU.mult,
+            )
+            return prod
+
+        def turn(prod_b, mu_b, out, engine):
+            bank = psum.tile([P, T, P], F32, name="tp", tag="tp", bufs=4)
+            for t in range(T):
+                nc.tensor.matmul(bank[:, t, :], lhsT=prod_b[:, t, :], rhs=ident_f[:], is_transpose=True, start=(t == 0), stop=False)
+            for t in range(T):
+                nc.tensor.matmul(bank[:, t, :], lhsT=mu_b[:, t::T], rhs=ident_b[:], start=False, stop=(t == T - 1))
+            copy_to(engine, out, bank[:].rearrange("w t r -> w r t"))
+
+        def turn_words(words, grp, t_pair, engine):
+            bank = psum.tile([P, 2, 2, P], F32, name="tp", tag="tp", bufs=4)
+            for a in range(2):
+                for u in range(2):
+                    nc.tensor.transpose(bank[:, a, u, :], words[:, a, u::2], ident_f[:])
+            out = grp[:, 256 * t_pair : 256 * t_pair + 256, :].rearrange("p c k -> p (c k)").bitcast(F32)
+            copy_to(engine, out.rearrange("p (a m u) -> p a m u", a=2, u=2), bank[:].rearrange("p a u m -> p a m u"))
+
+        w2c = {}
+        gc = {}
+        xc = []
+        w1c = {}
+        dzc = {}
+        dzt = {}
+
+        w2_const = {}
+
+        def build_w2(j, q, e, mult_engine="v", copy_engine="s"):
+            sg, mu = w2_const[q]
+            grp = grp_tile("w2g")
+            for r in range(2):
+                prod = multiply(mult_engine, e[:, 2 * r : 2 * r + 2, :], sg[:, 2 * r : 2 * r + 2, :])
+                for b in range(2):
+                    c0 = P * (2 * r + b)
+                    turn(prod[:, b], mu[:, 2 * r + b, :], grp[:, c0 : c0 + P, :], copy_engine)
+            c = code_tile("w2c", 512, "w2c", 3)
+            quantize(c, 0, 512, E4M3, grp[:].rearrange("p c k -> p (c k)"))
+            w2c[j, q] = c
+
+        def build_grad(j, g, gr, copy_engine="s"):
+            grp = grp_tile("gg")
+            words = gr[:].rearrange("p t y -> p (t y)").bitcast(F32).rearrange("p (t w) -> p t w", t=T)
+            for tp in range(2):
+                turn_words(words[:, 2 * tp : 2 * tp + 2, :], grp, tp, copy_engine)
+            c = code_tile("gc", 512, "gc", 3)
+            quantize(c, 0, 512, E5M2, grp[:].rearrange("p c k -> p (c k)"))
+            gc[j, g] = c
+
+        def build_x(g, half, xr, engine="v"):
+            if half == 0:
+                xc.append(code_tile("xc%d" % g, X, "xc%d" % g, 1))
+            grp = grp_tile("xg")
+            if engine == "g":
+                nc.gpsimd.tensor_scalar(out=grp[:], in0=xr[:].rearrange("p t w -> p w t"), scalar1=1.0, scalar2=0.0, op0=ALU.mult, op1=ALU.add)
+            else:
+                copy_to(engine, grp[:], xr[:].rearrange("p t w -> p w t"))
+            quantize(xc[g], 512 * half, 512 * half + 512, E4M3, grp[:].rearrange("p c k -> p (c k)"))
+
+        w1g = {}
+
+        def w1_steps(i, j, sg, es, mu, mult_engine, copy_engine="s"):
+            made = {}
+
+            def first():
+                if i == 0:
+                    for c in range(2):
+                        w1c[j, c] = code_tile("w1c%d%d" % (j, c), X, "w1c%d%d" % (j, c), 1)
+                made["prod"] = multiply(
+                    mult_engine, es[j][:].rearrange("p (b y) -> p b y", b=2), sg[:].rearrange("p (b y) -> p b y", b=2)
+                )
+
+            def second():
+                for c in range(2):
+                    if i % 4 == 0:
+                        w1g[j, c] = grp_tile("w1g")
+                    c0 = P * (i % 4)
+                    turn(made["prod"][:, c], mu[:, 512 * c : 512 * c + 512], w1g[j, c][:, c0 : c0 + P, :], copy_engine)
+
+            def third():
+                for c in range(2):
+                    h0 = 512 * (i // 4)
+                    quantize(w1c[j, c], h0, h0 + 512, E4M3, w1g[j, c][:].rearrange("p c k -> p (c k)"))
+
+            return [first, second] + ([third] if i % 4 == 3 else [])
+
+        def dz_steps(j, g, zs, inter_engines="ss", copy_engine="s"):
+            dz = {}
+            grp = {}
+
+            def absolute(t):
+                nc.scalar.activation(out=zs[t][:], in_=zs[t][:], func=ACT.Abs)
+
+            def mask(t):
+                for q in range(2):
+                    if t == 0:
+                        dz[q] = work.tile([P, T, 512], BF16, name="dz", tag="dz", bufs=4, align_bytes=64)
+                    bank = psum.tile([P, 512], F32, name="mm", tag="mm", bufs=4)
+                    nc.tensor.matmul_mx(
+                        out=bank[:],
+                        lhsT=gc[j, g][0][:, P * t : P * t + P].bitcast(E5M2),
+                        lhsT_scale=gc[j, g][1][:, P * t : P * t + P],
+                        rhs=w2c[j, q][0][:].bitcast(E4M3),
+                        rhs_scale=w2c[j, q][1][:],
+                        start=True,
+                        stop=True,
+                    )
+                    nc.vector.scalar_tensor_tensor(
+                        out=dz[q][:, t, :], in0=zs[t][:, 512 * q : 512 * q + 512], scalar=1.0, in1=bank[:], op0=ALU.is_lt, op1=ALU.mult
+                    )
+
+            def turn_pair(q, half):
+                if half == 0:
+                    grp[q] = grp_tile("dg")
+                words = dz[q][:].rearrange("p t y -> p (t y)").bitcast(F32).rearrange("p (t w) -> p t w", t=T)
+                turn_words(words[:, 2 * half : 2 * half + 2, :], grp[q], half, copy_engine)
+
+            def interleave(q):
+                if q == 0:
+                    dzc[j, g] = code_tile("dzc%d%d" % (j, g), H, "dzc%d%d" % (j, g), 1)
+                    dzt[j, g] = code_tile("dzt%d%d" % (j, g), H, "dzt%d%d" % (j, g), 1)
+                inter = grp_tile("di")
+                grp[2 + q] = inter
+                copy_to(inter_engines[q], inter[:], dz[q][:].rearrange("p t h -> p h t"))
+
+            def quant(q):
+                quantize(dzt[j, g], 512 * q, 512 * q + 512, E5M2, grp[q][:].rearrange("p c k -> p (c k)"))
+
+            def quant2(q):
+                quantize(dzc[j, g], 512 * q, 512 * q + 512, E5M2, grp[2 + q][:].rearrange("p c k -> p (c k)"))
+
+            return [
+                lambda: absolute(0),
+                lambda: absolute(1),
+                lambda: mask(0),
+                lambda: (absolute(2), mask(1)),
+                lambda: (turn_pair(0, 0), absolute(3), mask(2)),
+                lambda: turn_pair(1, 0),
+                lambda: mask(3),
+                lambda: turn_pair(0, 1),
+                lambda: interleave(0),
+                lambda: turn_pair(1, 1),
+                lambda: quant(0),
+                lambda: interleave(1),
+                lambda: (quant(1), quant2(0)),
+                lambda: quant2(1),
+            ]
+
+        def dx(g, t, copy_engine="s"):
+            ot = raw.tile([P, X], F32, name="ot", tag="in4", bufs=4)
+            for xh in range(2):
+                bank = psum.tile([P, 512], F32, name="mm", tag="mm", bufs=4)
+                for k in range(4):
+                    j, c = divmod(k, 2)
+                    cols = slice(512 * c + P * t, 512 * c + P * t + P)
+                    xcols = slice(512 * xh, 512 * xh + 512)
+                    nc.tensor.matmul_mx(
+                        out=bank[:],
+                        lhsT=dzt[j, g][0][:, cols].bitcast(E5M2),
+                        lhsT_scale=dzt[j, g][1][:, cols],
+                        rhs=w1c[j, c][0][:, xcols].bitcast(E4M3),
+                        rhs_scale=w1c[j, c][1][:, xcols],
+                        start=(k == 0),
+                        stop=(k == 3),
+                    )
+                copy_to(copy_engine, ot[:, 512 * xh : 512 * xh + 512], bank[:])
+            nc.sync.dma_start(out=out_0.rearrange("(g m t) x -> g t m x", g=2, t=T)[g, t], in_=ot[:])
+
+        def dw(i, es, add_engine="v"):
+            parts = []
+            for j in range(J):
+                part = raw.tile([P, H], F32, name="part", tag="w2s", bufs=4)
+                for hh in range(2):
+                    hc = slice(512 * hh, 512 * hh + 512)
+                    bank = psum.tile([P, 512], F32, name="mm", tag="mm", bufs=4)
+                    for g in range(2):
+                        nc.tensor.matmul_mx(
+                            out=bank[:],
+                            lhsT=xc[g][0][:, P * i : P * i + P].bitcast(E4M3),
+                            lhsT_scale=xc[g][1][:, P * i : P * i + P],
+                            rhs=dzc[j, g][0][:, hc].bitcast(E5M2),
+                            rhs_scale=dzc[j, g][1][:, hc],
+                            start=(g == 0),
+                            stop=(g == 1),
+                        )
+                    nc.vector.tensor_tensor(out=part[:, hc], in0=es[j][:, hc], in1=bank[:], op=ALU.mult)
+                parts.append(part)
+            eng = nc.gpsimd if add_engine == "g" else nc.vector
+            eng.tensor_tensor(out=parts[0][:], in0=parts[0][:], in1=parts[1][:], op=ALU.add)
+            nc.sync.dma_start(out=out_1[P * i : P * i + P, :], in_=parts[0][:])
+
+        def run(*lists):
+            order = []
+            for k in range(len(lists)):
+                n = len(lists[k])
+                for i in range(n):
+                    order.append(((i + 0.5) / n, k, i))
+            for at, k, i in sorted(order):
+                lists[k][i]()
+
+        e2 = {}
+        gr = {}
+        for q in range(2):
+            sg = raw.tile([P, 4, Y], BF16, name="sg2", tag="w2s", bufs=4)
+            nc.sync.dma_start(out=sg[:], in_=sig_W2.rearrange("(q b m) y -> q m b y", q=2, b=4)[q])
+            e2[0, q] = load_e2(0, q)
+            mu = raw.tile([P, 4, Y], BF16, name="mu2", tag="w2s", bufs=4)
+            nc.sync.dma_start(out=mu[:], in_=mu_W2.rearrange("(q b m) y -> q m b y", q=2, b=4)[q])
+            w2_const[q] = (sg, mu)
+            gr[0, q] = load_grad(0, q)
+        z00 = [load_z(0, 0, t) for t in range(T)]
+        w1 = {}
+        w1[0] = load_w1(0)
+        build_w2(0, 0, e2[0, 0])
+        build_grad(0, 0, gr[0, 0])
+        build_w2(0, 1, e2[0, 1])
+        build_grad(0, 1, gr[0, 1])
+        w1[1] = load_w1(1)
+
+        def w1_list(items, engines):
+            res = []
+            for i in items:
+                for j in range(J):
+                    res += w1_steps(i, j, w1[i][0], w1[i][1], w1[i][2], engines[j])
+            return res
+
+        w1[2] = load_w1(2)
+        z01 = [load_z(0, 1, t) for t in range(T)]
+        run(dz_steps(0, 0, z00, "vs"), w1_list([0, 1, 2], "vg"))
+        for i in range(3, 6):
+            w1[i] = load_w1(i)
+        for q in range(2):
+            e2[1, q] = load_e2(1, q)
+            gr[1, q] = load_grad(1, q)
+        run(dz_steps(0, 1, z01, "vs"), w1_list([3, 4, 5], "vg"))
+        z10 = [load_z(1, 0, t) for t in range(T)]
+        for i in range(6, 8):
+            w1[i] = load_w1(i)
+        for q in range(2):
+            build_w2(1, q, e2[1, q])
+            build_grad(1, q, gr[1, q])
+        xr = [load_x(0, 0), load_x(0, 1), load_x(1, 0), load_x(1, 1)]
+        run(dz_steps(1, 0, z10, "vs"), w1_list([6, 7], "vv"), [lambda: build_x(0, 0, xr[0], "g"), lambda: build_x(0, 1, xr[1], "g")])
+        z11 = [load_z(1, 1, t) for t in range(T)]
+        run(
+            dz_steps(1, 1, z11, "vs"),
+            [lambda: dx(0, 0), lambda: dx(0, 1), lambda: dx(0, 2), lambda: dx(0, 3)],
+            [lambda: build_x(1, 0, xr[2], "g"), lambda: build_x(1, 1, xr[3], "g")],
+        )
+        for i in range(8):
+            dw(i, w1[i][1], "g" if i % 2 == 0 and i < 7 else "v")
+            if i % 2 == 1:
+                dx(1, i // 2)

@@ -19,6 +19,14 @@ BYTES = 2 * (N * X + 2 * X * H + J * X * H + 2 * H * Y + J * H * Y + J * N * Y) 
 
 P = 128
 T = 4
+K = 512
+EDGE = 1.0 + 3.0 / 256.0
+SMALL_SLOTS = 34
+LARGE_SLOTS = 3
+CODE_SLOTS = 30
+LEAD = 6
+AHEAD = 2
+BEHIND = 3
 
 
 def tile_gaussian_nn_htanh_v_kernel(
@@ -27,338 +35,412 @@ def tile_gaussian_nn_htanh_v_kernel(
     nc = tc.nc
 
     with ExitStack() as ctx:
-        const = ctx.enter_context(tc.tile_pool(name="const", bufs=1))
-        raw = ctx.enter_context(tc.tile_pool(name="raw", bufs=2))
-        work = ctx.enter_context(tc.tile_pool(name="work", bufs=2))
-        codes = ctx.enter_context(tc.tile_pool(name="codes", bufs=1))
-        psum = ctx.enter_context(tc.psum_pool(name="psum", bufs=4))
+        sbuf = ctx.enter_context(tc.tile_pool(name="sbuf", bufs=1))
+        psum = ctx.enter_context(tc.psum_pool(name="psum", bufs=1))
 
-        ident_f = const.tile([P, P], F32, name="ident_f", tag="ident_f")
+        ident_f = sbuf.tile([P, P], F32, name="ident_f", tag="ident_f")
         make_identity(nc, ident_f[:])
-        ident_b = const.tile([P, P], BF16, name="ident_b", tag="ident_b")
+        ident_b = sbuf.tile([P, P], BF16, name="ident_b", tag="ident_b")
         nc.vector.tensor_copy(out=ident_b[:], in_=ident_f[:])
+        ctx.enter_context(tc.manual_schedule())
 
-        def copy_to(engine, out, in_):
-            if engine == "s":
-                nc.scalar.copy(out=out, in_=in_)
+        free = {
+            "small": list(range(SMALL_SLOTS)),
+            "large": list(range(LARGE_SLOTS)),
+            "code": list(range(CODE_SLOTS)),
+            "bank": list(range(8)),
+        }
+        held = {}
+        tiles = {}
+
+        def take(key, kind, shape, dtype):
+            slot = free[kind].pop(0)
+            held[key] = (kind, slot)
+            tag = "%s%d" % (kind, slot)
+            if kind == "bank":
+                tiles[key] = psum.tile(shape, dtype, name=key[0], tag=tag)
+            elif kind == "code":
+                words = sbuf.tile(shape, U32, name=key[0], tag=tag, align_bytes=64)
+                scales = sbuf.tile(shape, U8, name=key[0] + "_s", tag=tag + "_s", align_bytes=64)
+                tiles[key] = (words, scales)
             else:
-                nc.vector.tensor_copy(out=out, in_=in_)
+                tiles[key] = sbuf.tile(shape, dtype, name=key[0], tag=tag, align_bytes=64)
+            return tiles[key]
 
-        def code_tile(name, width, tag, bufs):
-            c = codes.tile([P, width], U32, name=name, tag=tag, bufs=bufs, align_bytes=64)
-            s = codes.tile([P, width], U8, name=name + "_s", tag=tag + "_s", bufs=bufs, align_bytes=64)
-            return c, s
+        def give(*keys):
+            for key in keys:
+                kind, slot = held.pop(key)
+                free[kind].append(slot)
 
-        def quantize(dst, c0, c1, fmt, src):
-            nc.vector.quantize_mx(out=dst[0][:, c0:c1].bitcast(fmt), scales=dst[1][:, c0:c1], in_=src)
+        def load(key, kind, shape, dtype, src):
+            nc.sync.dma_start(out=take(key, kind, shape, dtype)[:], in_=src)
 
-        def grp_tile(name):
-            return work.tile([P, 512, T], BF16, name=name, tag="grp", bufs=6, align_bytes=64)
+        def quantize(key, fmt, src_key):
+            words, scales = take(key, "code", [P, K], U32)
+            src = tiles[src_key][:].rearrange("p c t -> p (c t)")
+            nc.vector.quantize_mx(out=words[:].bitcast(fmt), scales=scales[:], in_=src)
 
-        def load_w2_const(q):
-            v = sig_W2.rearrange("(q b m) y -> q m b y", q=2, b=4)
-            sg = raw.tile([P, 4, Y], BF16, name="sg2", tag="w2s", bufs=4)
-            nc.sync.dma_start(out=sg[:], in_=v[q])
-            v = mu_W2.rearrange("(q b m) y -> q m b y", q=2, b=4)
-            mu = raw.tile([P, 4, Y], BF16, name="mu2", tag="w2s", bufs=4)
-            nc.sync.dma_start(out=mu[:], in_=v[q])
-            return sg, mu
-
-        def load_e2(j, q):
-            v = e_W2[j].rearrange("(q b m) y -> q m b y", q=2, b=4)
-            e = raw.tile([P, 4, Y], BF16, name="e2", tag="in4", bufs=4)
-            nc.sync.dma_start(out=e[:], in_=v[q])
-            return e
-
-        def load_grad(j, g):
-            v = grad_out[j].rearrange("(g p t) y -> g p t y", g=2, t=T)
-            t = raw.tile([P, T, Y], BF16, name="gr", tag="in4", bufs=4)
-            nc.sync.dma_start(out=t[:], in_=v[g])
-            return t
-
-        def load_x(g, half):
-            v = x.rearrange("(g p t) w -> g p t w", g=2, t=T)
-            t = raw.tile([P, T, 512], BF16, name="xr", tag="in4", bufs=4)
-            nc.sync.dma_start(out=t[:], in_=v[g][:, :, 512 * half : 512 * half + 512])
-            return t
-
-        def load_z(j, g, t):
-            v = z1[j].rearrange("(g p t) h -> g t p h", g=2, t=T)
-            zt = raw.tile([P, H], F32, name="z", tag="z", bufs=4)
-            nc.sync.dma_start(out=zt[:], in_=v[g, t])
-            return zt
-
-        def load_w1(i):
-            rows = slice(P * i, P * i + P)
-            sg = raw.tile([P, H], BF16, name="sg1", tag="sg1", bufs=3)
-            nc.sync.dma_start(out=sg[:], in_=sig_W1[rows, :])
-            es = []
-            for j in range(J):
-                e = raw.tile([P, H], BF16, name="e1", tag="e1", bufs=16)
-                nc.sync.dma_start(out=e[:], in_=e_W1[j][rows, :])
-                es.append(e)
-            mu = raw.tile([P, H], BF16, name="mu1", tag="mu1", bufs=3)
-            nc.sync.dma_start(out=mu[:], in_=mu_W1[rows, :])
-            return sg, es, mu
-
-        def multiply(engine, e, sg):
-            prod = work.tile([P, 2, T, P], F32, name="prod", tag="prod", bufs=3)
-            eng = nc.gpsimd if engine == "g" else nc.vector
-            eng.tensor_tensor(
-                out=prod[:],
-                in0=e.rearrange("p b (w t) -> p b t w", t=T),
-                in1=sg.rearrange("p b (w t) -> p b t w", t=T),
-                op=ALU.mult,
+        def mx(bank, lhs_key, lhs_cols, lhs_fmt, rhs_key, rhs_cols, rhs_fmt, start, stop):
+            lhs, rhs = tiles[lhs_key], tiles[rhs_key]
+            nc.tensor.matmul_mx(
+                out=bank,
+                lhsT=lhs[0][:, lhs_cols].bitcast(lhs_fmt),
+                lhsT_scale=lhs[1][:, lhs_cols],
+                rhs=rhs[0][:, rhs_cols].bitcast(rhs_fmt),
+                rhs_scale=rhs[1][:, rhs_cols],
+                start=start,
+                stop=stop,
             )
-            return prod
 
-        def turn(prod_b, mu_b, out, engine):
-            bank = psum.tile([P, T, P], F32, name="tp", tag="tp", bufs=4)
+        def cols(n, width=P):
+            return slice(width * n, width * n + width)
+
+        def turn_sum(bank, mean_of, prod_of):
             for t in range(T):
-                nc.tensor.matmul(bank[:, t, :], lhsT=prod_b[:, t, :], rhs=ident_f[:], is_transpose=True, start=(t == 0), stop=False)
+                nc.tensor.matmul(bank[:, t, :], lhsT=mean_of(t), rhs=ident_b[:], start=(t == 0), stop=False)
             for t in range(T):
-                nc.tensor.matmul(bank[:, t, :], lhsT=mu_b[:, t::T], rhs=ident_b[:], start=False, stop=(t == T - 1))
-            copy_to(engine, out, bank[:].rearrange("w t r -> w r t"))
+                nc.tensor.matmul(bank[:, t, :], lhsT=prod_of(t), rhs=ident_f[:], is_transpose=True, start=False, stop=(t == T - 1))
 
-        def turn_words(words, grp, t_pair, engine):
-            bank = psum.tile([P, 2, 2, P], F32, name="tp", tag="tp", bufs=4)
-            for a in range(2):
-                for u in range(2):
-                    nc.tensor.transpose(bank[:, a, u, :], words[:, a, u::2], ident_f[:])
-            out = grp[:, 256 * t_pair : 256 * t_pair + 256, :].rearrange("p c k -> p (c k)").bitcast(F32)
-            copy_to(engine, out.rearrange("p (a m u) -> p a m u", a=2, u=2), bank[:].rearrange("p a u m -> p a m u"))
+        READ, QUANT, MAKE, PE, DMA = 1, 2, 3, 0, 4
 
-        w2c = {}
-        gc = {}
-        xc = []
-        w1c = {}
-        dzc = {}
-        dzt = {}
+        def w2_job(j, q, r):
+            def fetch():
+                if j == 0:
+                    load(("sig2", q, r), "small", [P, 2, Y], BF16, sig_W2.rearrange("(a b m) y -> a m b y", b=2, m=P)[2 * q + r])
+                load(("e2", j, q, r), "small", [P, 2, Y], BF16, e_W2[j].rearrange("(a b m) y -> a m b y", b=2, m=P)[2 * q + r])
+                if j == 0:
+                    load(("mu2", q, r), "small", [P, 2, Y], BF16, mu_W2.rearrange("(a b m) y -> a m b y", b=2, m=P)[2 * q + r])
 
-        w2_const = {}
+            def sort_mean():
+                dst = take(("mean2", q, r), "small", [P, 2, T, P], BF16)
+                nc.scalar.copy(out=dst[:], in_=tiles["mu2", q, r][:].rearrange("p b (w t) -> p b t w", t=T))
+                give(("mu2", q, r))
 
-        def build_w2(j, q, e, mult_engine="v", copy_engine="s"):
-            sg, mu = w2_const[q]
-            grp = grp_tile("w2g")
-            for r in range(2):
-                prod = multiply(mult_engine, e[:, 2 * r : 2 * r + 2, :], sg[:, 2 * r : 2 * r + 2, :])
-                for b in range(2):
-                    c0 = P * (2 * r + b)
-                    turn(prod[:, b], mu[:, 2 * r + b, :], grp[:, c0 : c0 + P, :], copy_engine)
-            c = code_tile("w2c", 512, "w2c", 3)
-            quantize(c, 0, 512, E4M3, grp[:].rearrange("p c k -> p (c k)"))
-            w2c[j, q] = c
-
-        def build_grad(j, g, gr, copy_engine="s"):
-            grp = grp_tile("gg")
-            words = gr[:].rearrange("p t y -> p (t y)").bitcast(F32).rearrange("p (t w) -> p t w", t=T)
-            for tp in range(2):
-                turn_words(words[:, 2 * tp : 2 * tp + 2, :], grp, tp, copy_engine)
-            c = code_tile("gc", 512, "gc", 3)
-            quantize(c, 0, 512, E5M2, grp[:].rearrange("p c k -> p (c k)"))
-            gc[j, g] = c
-
-        def build_x(g, half, xr, engine="v"):
-            if half == 0:
-                xc.append(code_tile("xc%d" % g, X, "xc%d" % g, 1))
-            grp = grp_tile("xg")
-            if engine == "g":
-                nc.gpsimd.tensor_scalar(out=grp[:], in0=xr[:].rearrange("p t w -> p w t"), scalar1=1.0, scalar2=0.0, op0=ALU.mult, op1=ALU.add)
-            else:
-                copy_to(engine, grp[:], xr[:].rearrange("p t w -> p w t"))
-            quantize(xc[g], 512 * half, 512 * half + 512, E4M3, grp[:].rearrange("p c k -> p (c k)"))
-
-        w1g = {}
-
-        def w1_steps(i, j, sg, es, mu, mult_engine, copy_engine="s"):
-            made = {}
-
-            def first():
-                if i == 0:
-                    for c in range(2):
-                        w1c[j, c] = code_tile("w1c%d%d" % (j, c), X, "w1c%d%d" % (j, c), 1)
-                made["prod"] = multiply(
-                    mult_engine, es[j][:].rearrange("p (b y) -> p b y", b=2), sg[:].rearrange("p (b y) -> p b y", b=2)
+            def multiply():
+                prod = take(("prod2", j, q, r), "small", [P, 2, T, P], F32)
+                order = "p b (w t) -> p b t w"
+                nc.vector.tensor_tensor(
+                    out=prod[:],
+                    in0=tiles["e2", j, q, r][:].rearrange(order, t=T),
+                    in1=tiles["sig2", q, r][:].rearrange(order, t=T),
+                    op=ALU.mult,
                 )
+                give(("e2", j, q, r))
+                if j == J - 1:
+                    give(("sig2", q, r))
 
-            def second():
-                for c in range(2):
-                    if i % 4 == 0:
-                        w1g[j, c] = grp_tile("w1g")
-                    c0 = P * (i % 4)
-                    turn(made["prod"][:, c], mu[:, 512 * c : 512 * c + 512], w1g[j, c][:, c0 : c0 + P, :], copy_engine)
+            def turn():
+                prod, mu = tiles["prod2", j, q, r], tiles["mean2", q, r]
+                for b in range(2):
+                    bank = take(("w2bank", j, q, r, b), "bank", [P, T, P], F32)
+                    turn_sum(bank, lambda t: mu[:, b, t, :], lambda t: prod[:, b, t, :])
+                give(("prod2", j, q, r))
+                if j == J - 1:
+                    give(("mean2", q, r))
 
-            def third():
-                for c in range(2):
-                    h0 = 512 * (i // 4)
-                    quantize(w1c[j, c], h0, h0 + 512, E4M3, w1g[j, c][:].rearrange("p c k -> p (c k)"))
+            def empty():
+                if r == 0:
+                    take(("w2in", j, q), "small", [P, K, T], BF16)
+                dst = tiles["w2in", j, q][:].rearrange("p (u b i) t -> p u b i t", u=T, i=8)
+                for b in range(2):
+                    blocks = cols(2 * r + b, 4)
+                    src = tiles["w2bank", j, q, r, b][:].rearrange("p t (b u i) -> p u b i t", u=T, i=8)
+                    nc.scalar.copy(out=dst[:, :, blocks, :, :], in_=src)
+                    give(("w2bank", j, q, r, b))
 
-            return [first, second] + ([third] if i % 4 == 3 else [])
+            def quant():
+                quantize(("w2", j, q), E4M3, ("w2in", j, q))
+                give(("w2in", j, q))
 
-        def dz_steps(j, g, zs, inter_engines="ss", copy_engine="s"):
-            dz = {}
-            grp = {}
+            steps = [(-LEAD - AHEAD, DMA, fetch), (-AHEAD, MAKE, multiply), (0, PE, turn), (1, READ, empty)]
+            if j == 0:
+                steps.append((-AHEAD, MAKE, sort_mean))
+            return steps + ([(BEHIND, QUANT, quant)] if r == 1 else [])
 
-            def absolute(t):
-                nc.scalar.activation(out=zs[t][:], in_=zs[t][:], func=ACT.Abs)
+        def grad_job(j, g):
+            def fetch():
+                load(("grad", j, g), "small", [P, T, Y], BF16, grad_out[j].rearrange("(g p t) y -> g p t y", g=2, t=T)[g])
 
-            def mask(t):
+            def turn():
+                words = tiles["grad", j, g][:].rearrange("p t y -> p (t y)").bitcast(F32).rearrange("p (t w) -> p t w", t=T)
+                for a in range(2):
+                    bank = take(("gbank", j, g, a), "bank", [P, 2, 2, P], F32)
+                    for s in range(2):
+                        for u in range(2):
+                            nc.tensor.transpose(bank[:, s, u, :], words[:, 2 * a + s, u::2], ident_f[:])
+                give(("grad", j, g))
+
+            def empty():
+                dst = take(("gin", j, g), "small", [P, K, T], BF16)[:].rearrange("p c t -> p (c t)").bitcast(F32)
+                for a in range(2):
+                    out = dst[:, cols(a, K)].rearrange("p (s m u) -> p s m u", s=2, u=2)
+                    nc.scalar.copy(out=out, in_=tiles["gbank", j, g, a][:].rearrange("p s u m -> p s m u"))
+                    give(("gbank", j, g, a))
+
+            def quant():
+                quantize(("g", j, g), E5M2, ("gin", j, g))
+                give(("gin", j, g))
+
+            return [(-LEAD, DMA, fetch), (0, PE, turn), (1, READ, empty), (BEHIND, QUANT, quant)]
+
+        def x_job(g, half, engine):
+            def fetch():
+                load(("x", g), "large", [P, T, X], BF16, x.rearrange("(g p t) w -> g p t w", g=2, t=T)[g])
+
+            def interleave():
+                dst = take(("xin", g, half), "small", [P, K, T], BF16)
+                src = tiles["x", g][:, :, cols(half, K)].rearrange("p t w -> p w t")
+                if engine == "s":
+                    nc.scalar.copy(out=dst[:], in_=src)
+                else:
+                    nc.vector.tensor_copy(out=dst[:], in_=src)
+                if half == 1:
+                    give(("x", g))
+
+            def quant():
+                quantize(("xq", g, half), E4M3, ("xin", g, half))
+                give(("xin", g, half))
+
+            steps = [(0, MAKE, interleave), (BEHIND, QUANT, quant)]
+            return steps + ([(-LEAD - AHEAD, DMA, fetch)] if half == 0 else [])
+
+        def w1_job(i, j, engine):
+            a, r = divmod(i, 2)
+            xh, c = divmod(i, 4)
+            order = "p (b t i) -> p t b i"
+
+            def fetch():
+                if r == 0:
+                    load(("sig1", a), "small", [P, 2, H], BF16, sig_W1.rearrange("(a r m) h -> a m r h", r=2, m=P)[a])
+                load(("e1", i), "small", [P, J, H], BF16, e_W1[:, cols(i), :].rearrange("j m h -> m j h"))
+                if r == 0:
+                    load(("mu1", a), "small", [P, 2, H], BF16, mu_W1.rearrange("(a r m) h -> a m r h", r=2, m=P)[a])
+
+            def sort_mean():
+                dst = take(("mean1", a), "small", [P, 2, T, 32, 8], BF16)
+                nc.vector.tensor_copy(out=dst[:], in_=tiles["mu1", a][:].rearrange("p r (b t i) -> p r t b i", t=T, i=8))
+                give(("mu1", a))
+
+            def multiply():
+                prod = take(("prod1", i, j), "small", [P, T, 32, 8], F32)
+                eng = nc.gpsimd if engine == "g" else nc.vector
+                eng.tensor_tensor(
+                    out=prod[:],
+                    in0=tiles["e1", i][:, j, :].rearrange(order, t=T, i=8),
+                    in1=tiles["sig1", a][:, r, :].rearrange(order, t=T, i=8),
+                    op=ALU.mult,
+                )
+                if r == 1 and j == J - 1:
+                    give(("sig1", a))
+
+            def turn():
+                prod = tiles["prod1", i, j][:].rearrange("p t (q b) i -> p t q (b i)", q=2)
+                mean = tiles["mean1", a][:, r].rearrange("p t (q b) i -> p t q (b i)", q=2)
                 for q in range(2):
-                    if t == 0:
-                        dz[q] = work.tile([P, T, 512], BF16, name="dz", tag="dz", bufs=4, align_bytes=64)
-                    bank = psum.tile([P, 512], F32, name="mm", tag="mm", bufs=4)
-                    nc.tensor.matmul_mx(
-                        out=bank[:],
-                        lhsT=gc[j, g][0][:, P * t : P * t + P].bitcast(E5M2),
-                        lhsT_scale=gc[j, g][1][:, P * t : P * t + P],
-                        rhs=w2c[j, q][0][:].bitcast(E4M3),
-                        rhs_scale=w2c[j, q][1][:],
-                        start=True,
-                        stop=True,
-                    )
-                    nc.vector.scalar_tensor_tensor(
-                        out=dz[q][:, t, :], in0=zs[t][:, 512 * q : 512 * q + 512], scalar=1.0, in1=bank[:], op0=ALU.is_lt, op1=ALU.mult
-                    )
+                    bank = take(("w1bank", i, j, q), "bank", [P, T, P], F32)
+                    turn_sum(bank, lambda t: mean[:, t, q, :], lambda t: prod[:, t, q, :])
+                give(("prod1", i, j))
+                if r == 1 and j == J - 1:
+                    give(("mean1", a))
 
-            def turn_pair(q, half):
-                if half == 0:
-                    grp[q] = grp_tile("dg")
-                words = dz[q][:].rearrange("p t y -> p (t y)").bitcast(F32).rearrange("p (t w) -> p t w", t=T)
-                turn_words(words[:, 2 * half : 2 * half + 2, :], grp[q], half, copy_engine)
-
-            def interleave(q):
-                if q == 0:
-                    dzc[j, g] = code_tile("dzc%d%d" % (j, g), H, "dzc%d%d" % (j, g), 1)
-                    dzt[j, g] = code_tile("dzt%d%d" % (j, g), H, "dzt%d%d" % (j, g), 1)
-                inter = grp_tile("di")
-                grp[2 + q] = inter
-                copy_to(inter_engines[q], inter[:], dz[q][:].rearrange("p t h -> p h t"))
+            def empty():
+                for q in range(2):
+                    if c == 0:
+                        take(("w1in", j, q, xh), "small", [P, K, T], BF16)
+                    src = tiles["w1bank", i, j, q][:].rearrange("p t m -> p m t")
+                    nc.scalar.copy(out=tiles["w1in", j, q, xh][:, cols(c), :], in_=src)
+                    give(("w1bank", i, j, q))
 
             def quant(q):
-                quantize(dzt[j, g], 512 * q, 512 * q + 512, E5M2, grp[q][:].rearrange("p c k -> p (c k)"))
+                quantize(("w1", j, q, xh), E4M3, ("w1in", j, q, xh))
+                give(("w1in", j, q, xh))
 
-            def quant2(q):
-                quantize(dzc[j, g], 512 * q, 512 * q + 512, E5M2, grp[2 + q][:].rearrange("p c k -> p (c k)"))
+            steps = [(-AHEAD, MAKE, multiply), (0, PE, turn), (1, READ, empty)]
+            if j == 0:
+                steps.append((-LEAD - AHEAD, DMA, fetch))
+                if r == 0:
+                    steps.append((-AHEAD - 1, MAKE, sort_mean))
+            if c == 3:
+                steps += [(BEHIND, QUANT, lambda: quant(0)), (BEHIND + 1, QUANT, lambda: quant(1))]
+            return steps
 
-            return [
-                lambda: absolute(0),
-                lambda: absolute(1),
-                lambda: mask(0),
-                lambda: (absolute(2), mask(1)),
-                lambda: (turn_pair(0, 0), absolute(3), mask(2)),
-                lambda: turn_pair(1, 0),
-                lambda: mask(3),
-                lambda: turn_pair(0, 1),
-                lambda: interleave(0),
-                lambda: turn_pair(1, 1),
-                lambda: quant(0),
-                lambda: interleave(1),
-                lambda: (quant(1), quant2(0)),
-                lambda: quant2(1),
-            ]
+        def dh_job(j, q, g, half):
+            key = (j, q, g)
 
-        def dx(g, t, copy_engine="s"):
-            ot = raw.tile([P, X], F32, name="ot", tag="in4", bufs=4)
-            for xh in range(2):
-                bank = psum.tile([P, 512], F32, name="mm", tag="mm", bufs=4)
+            def fetch():
+                load(("z",) + key, "large", [P, T, K], F32, z1[j].rearrange("(g p t) h -> g p t h", g=2, t=T)[g][:, :, cols(q, K)])
+
+            def absolute():
+                if half == 0:
+                    take(("abs",) + key, "small", [P, K, T], BF16)
+                dst = tiles[("abs",) + key][:].rearrange("p (b v i) t -> p v b i t", v=2, i=16)
+                src = tiles[("z",) + key][:].rearrange("p t (b v i) -> p v b i t", v=2, i=16)
+                nc.scalar.activation(out=dst[:, half], in_=src[:, half], func=ACT.Abs, scale=EDGE)
+                if half == 1:
+                    give(("z",) + key)
+
+            def multiply():
+                for u in (2 * half, 2 * half + 1):
+                    bank = take(("dh",) + key + (u,), "bank", [P, T, P], F32)
+                    for t in range(T):
+                        mx(bank[:, t, :], ("g", j, g), cols(t), E5M2, ("w2", j, q), cols(u), E4M3, True, True)
+                if half == 1 and q == 1:
+                    give(("g", j, g))
+                if half == 1 and g == 1:
+                    give(("w2", j, q))
+
+            def mask():
+                if half == 0:
+                    take(("dz",) + key, "small", [P, K, T], BF16)
+                size = tiles[("abs",) + key][:].rearrange("p (b u i) t -> p u b i t", u=T, i=8)
+                dz = tiles[("dz",) + key][:].rearrange("p (u b i) t -> p u b i t", u=T, i=8)
+                for u in (2 * half, 2 * half + 1):
+                    bank = tiles[("dh",) + key + (u,)][:].rearrange("p t (b i) -> p b i t", i=8)
+                    nc.vector.scalar_tensor_tensor(out=dz[:, u], in0=size[:, u], scalar=EDGE, in1=bank, op0=ALU.is_lt, op1=ALU.mult)
+                    give(("dh",) + key + (u,))
+                if half == 1:
+                    give(("abs",) + key)
+
+            steps = [(-AHEAD, MAKE, absolute), (0, PE, multiply), (1, READ, mask)]
+            if half == 0:
+                steps += [(-LEAD - AHEAD, DMA, fetch)]
+            return steps
+
+        def dzt_job(j, q, g):
+            key = (j, q, g)
+
+            def turn():
+                words = tiles[("dz",) + key][:].rearrange("p c t -> p (c t)").bitcast(F32).rearrange("p (u m s) -> p u m s", u=T, s=2)
+                for s in range(2):
+                    bank = take(("dzbank",) + key + (s,), "bank", [P, T, P], F32)
+                    for u in range(T):
+                        nc.tensor.transpose(bank[:, u, :], words[:, u, :, s], ident_f[:])
+                give(("dz",) + key)
+
+            def quant_tokens():
+                quantize(("dzn",) + key, E5M2, ("dz",) + key)
+
+            def empty():
+                dst = take(("dzin",) + key, "small", [P, K, T], BF16)
+                for s in range(2):
+                    src = tiles[("dzbank",) + key + (s,)][:].bitcast(BF16).rearrange("p u (m e) -> p e m u", e=2)
+                    nc.scalar.copy(out=dst[:, cols(s, 256), :].rearrange("p (e m) u -> p e m u", e=2), in_=src)
+                    give(("dzbank",) + key + (s,))
+
+            def quant_features():
+                quantize(("dzh",) + key, E5M2, ("dzin",) + key)
+                give(("dzin",) + key)
+
+            return [(0, PE, turn), (-1, QUANT, quant_tokens), (1, READ, empty), (BEHIND, QUANT, quant_features)]
+
+        def dx_job(g, xh, t):
+            pair = (g, xh, t // 2)
+
+            def multiply():
+                bank = take(("dx", g, xh, t), "bank", [P, K], F32)
                 for k in range(4):
-                    j, c = divmod(k, 2)
-                    cols = slice(512 * c + P * t, 512 * c + P * t + P)
-                    xcols = slice(512 * xh, 512 * xh + 512)
-                    nc.tensor.matmul_mx(
-                        out=bank[:],
-                        lhsT=dzt[j, g][0][:, cols].bitcast(E5M2),
-                        lhsT_scale=dzt[j, g][1][:, cols],
-                        rhs=w1c[j, c][0][:, xcols].bitcast(E4M3),
-                        rhs_scale=w1c[j, c][1][:, xcols],
-                        start=(k == 0),
-                        stop=(k == 3),
-                    )
-                copy_to(copy_engine, ot[:, 512 * xh : 512 * xh + 512], bank[:])
-            nc.sync.dma_start(out=out_0.rearrange("(g m t) x -> g t m x", g=2, t=T)[g, t], in_=ot[:])
+                    j, q = divmod(k, 2)
+                    mx(bank[:], ("dzh", j, q, g), cols(t), E5M2, ("w1", j, q, xh), cols(0, K), E4M3, k == 0, k == 3)
+                    if t == T - 1 and xh == 1:
+                        give(("dzh", j, q, g))
+                    if t == T - 1 and g == 1:
+                        give(("w1", j, q, xh))
 
-        def dw(i, es, add_engine="v"):
-            parts = []
-            for j in range(J):
-                part = raw.tile([P, H], F32, name="part", tag="w2s", bufs=4)
-                for hh in range(2):
-                    hc = slice(512 * hh, 512 * hh + 512)
-                    bank = psum.tile([P, 512], F32, name="mm", tag="mm", bufs=4)
+            def empty():
+                if t % 2 == 0:
+                    take(("out0",) + pair, "small", [P, 2, K], F32)
+                nc.scalar.copy(out=tiles[("out0",) + pair][:, t % 2, :], in_=tiles["dx", g, xh, t][:])
+                give(("dx", g, xh, t))
+
+            def store():
+                dst = out_0.rearrange("(g p t) w -> g p t w", g=2, t=T)[g][:, cols(t // 2, 2), cols(xh, K)]
+                nc.sync.dma_start(out=dst, in_=tiles[("out0",) + pair][:])
+                give(("out0",) + pair)
+
+            return [(0, PE, multiply), (1, READ, empty)] + ([(1, DMA, store)] if t % 2 == 1 else [])
+
+        def dw_job(q, items, engine):
+            def multiply():
+                for i, j in items:
+                    bank = take(("dw", q, i, j), "bank", [P, K], F32)
                     for g in range(2):
-                        nc.tensor.matmul_mx(
-                            out=bank[:],
-                            lhsT=xc[g][0][:, P * i : P * i + P].bitcast(E4M3),
-                            lhsT_scale=xc[g][1][:, P * i : P * i + P],
-                            rhs=dzc[j, g][0][:, hc].bitcast(E5M2),
-                            rhs_scale=dzc[j, g][1][:, hc],
-                            start=(g == 0),
-                            stop=(g == 1),
-                        )
-                    nc.vector.tensor_tensor(out=part[:, hc], in0=es[j][:, hc], in1=bank[:], op=ALU.mult)
-                parts.append(part)
-            eng = nc.gpsimd if add_engine == "g" else nc.vector
-            eng.tensor_tensor(out=parts[0][:], in0=parts[0][:], in1=parts[1][:], op=ALU.add)
-            nc.sync.dma_start(out=out_1[P * i : P * i + P, :], in_=parts[0][:])
+                        mx(bank[:], ("xq", g, i // 4), cols(i % 4), E4M3, ("dzn", j, q, g), cols(0, K), E5M2, g == 0, g == 1)
+                        if i == 7:
+                            give(("dzn", j, q, g))
 
-        def run(*lists):
-            order = []
-            for k in range(len(lists)):
-                n = len(lists[k])
-                for i in range(n):
-                    order.append(((i + 0.5) / n, k, i))
-            for at, k, i in sorted(order):
-                lists[k][i]()
+            def weigh():
+                for i, j in items:
+                    if i % 2 == 0:
+                        take(("part", q, i // 2, j), "small", [P, 2, K], F32)
+                    nc.vector.tensor_tensor(
+                        out=tiles["part", q, i // 2, j][:, i % 2, :].rearrange("p (b u i) -> p b u i", u=T, i=8),
+                        in0=tiles["e1", i][:, j, cols(q, K)].rearrange("p (b u i) -> p b u i", u=T, i=8),
+                        in1=tiles["dw", q, i, j][:].rearrange("p (u b i) -> p b u i", u=T, i=8),
+                        op=ALU.mult,
+                    )
+                    give(("dw", q, i, j))
+                    if q == 1 and j == J - 1:
+                        give(("e1", i))
 
-        e2 = {}
-        gr = {}
-        for q in range(2):
-            sg = raw.tile([P, 4, Y], BF16, name="sg2", tag="w2s", bufs=4)
-            nc.sync.dma_start(out=sg[:], in_=sig_W2.rearrange("(q b m) y -> q m b y", q=2, b=4)[q])
-            e2[0, q] = load_e2(0, q)
-            mu = raw.tile([P, 4, Y], BF16, name="mu2", tag="w2s", bufs=4)
-            nc.sync.dma_start(out=mu[:], in_=mu_W2.rearrange("(q b m) y -> q m b y", q=2, b=4)[q])
-            w2_const[q] = (sg, mu)
-            gr[0, q] = load_grad(0, q)
-        z00 = [load_z(0, 0, t) for t in range(T)]
-        w1 = {}
-        w1[0] = load_w1(0)
-        build_w2(0, 0, e2[0, 0])
-        build_grad(0, 0, gr[0, 0])
-        build_w2(0, 1, e2[0, 1])
-        build_grad(0, 1, gr[0, 1])
-        w1[1] = load_w1(1)
+            def add(i):
+                first, second = tiles["part", q, i // 2, 0][:, i % 2, :], tiles["part", q, i // 2, 1][:, i % 2, :]
+                eng = nc.gpsimd if engine == "g" else nc.vector
+                eng.tensor_tensor(out=first, in0=first, in1=second, op=ALU.add)
+                if i % 2 == 1:
+                    give(("part", q, i // 2, 1))
 
-        def w1_list(items, engines):
-            res = []
-            for i in items:
-                for j in range(J):
-                    res += w1_steps(i, j, w1[i][0], w1[i][1], w1[i][2], engines[j])
-            return res
+            def store(i):
+                dst = out_1.rearrange("(a r m) h -> a m r h", r=2, m=P)[i // 2][:, :, cols(q, K)]
+                nc.sync.dma_start(out=dst, in_=tiles["part", q, i // 2, 0][:])
+                give(("part", q, i // 2, 0))
 
-        w1[2] = load_w1(2)
-        z01 = [load_z(0, 1, t) for t in range(T)]
-        run(dz_steps(0, 0, z00, "vs"), w1_list([0, 1, 2], "vg"))
-        for i in range(3, 6):
-            w1[i] = load_w1(i)
-        for q in range(2):
-            e2[1, q] = load_e2(1, q)
-            gr[1, q] = load_grad(1, q)
-        run(dz_steps(0, 1, z01, "vs"), w1_list([3, 4, 5], "vg"))
-        z10 = [load_z(1, 0, t) for t in range(T)]
-        for i in range(6, 8):
-            w1[i] = load_w1(i)
-        for q in range(2):
-            build_w2(1, q, e2[1, q])
-            build_grad(1, q, gr[1, q])
-        xr = [load_x(0, 0), load_x(0, 1), load_x(1, 0), load_x(1, 1)]
-        run(dz_steps(1, 0, z10, "vs"), w1_list([6, 7], "vv"), [lambda: build_x(0, 0, xr[0], "g"), lambda: build_x(0, 1, xr[1], "g")])
-        z11 = [load_z(1, 1, t) for t in range(T)]
-        run(
-            dz_steps(1, 1, z11, "vs"),
-            [lambda: dx(0, 0), lambda: dx(0, 1), lambda: dx(0, 2), lambda: dx(0, 3)],
-            [lambda: build_x(1, 0, xr[2], "g"), lambda: build_x(1, 1, xr[3], "g")],
-        )
-        for i in range(8):
-            dw(i, w1[i][1], "g" if i % 2 == 0 and i < 7 else "v")
-            if i % 2 == 1:
-                dx(1, i // 2)
+            done = [i for i, j in items if j == J - 1]
+            steps = [(0, PE, multiply), (1, READ, weigh), (1, MAKE, lambda: [add(i) for i in done])]
+            return steps + [(1, DMA, lambda: [store(i) for i in done if i % 2 == 1])]
+
+        def w2_jobs(j, q):
+            return [w2_job(j, q, r) for r in range(2)]
+
+        def w1_jobs(rows):
+            return [w1_job(i, j, "v") for i in rows for j in range(J)]
+
+        def dx_jobs(g, xh):
+            return [dx_job(g, xh, t) for t in range(T)]
+
+        def unit(key, last, side):
+            turn = [dzt_job(*last)] if last else []
+            n = len(side) // 2
+            return [dh_job(*key, 0)] + side[:1] + turn + side[1:n] + [dh_job(*key, 1)] + side[n:]
+
+        def weave(first, second):
+            jobs = []
+            for n in range(max(len(first), len(second))):
+                jobs += first[n : n + 1] + second[n : n + 1]
+            return jobs
+
+        order = [(j, q, g) for g in range(2) for q in range(2) for j in range(J)]
+        first = dx_jobs(0, 0) + dx_jobs(0, 1)
+        first = dx_jobs(0, 0) + dx_jobs(0, 1)
+        sides = [
+            w2_jobs(0, 1) + w2_jobs(1, 1),
+            w1_jobs([0, 1]),
+            w1_jobs([2, 3]),
+            [grad_job(0, 1)] + w1_jobs([4, 5]),
+            [grad_job(1, 1)] + w1_jobs([6, 7]) + [x_job(0, 0, "v")],
+            weave([x_job(0, 1, "s"), x_job(1, 0, "v"), x_job(1, 1, "v")], first[:6]),
+            first[6:7] + [dw_job(0, [(i, 0), (i, 1)], "g") for i in range(7)],
+            first[7:] + [dw_job(0, [(7, 0), (7, 1)], "g")] + [dw_job(1, [(i, 0), (i + 1, 0)], "g") for i in range(0, 4, 2)],
+        ]
+        jobs = w2_jobs(0, 0) + [grad_job(0, 0)] + w2_jobs(1, 0) + [grad_job(1, 0)]
+        for n in range(8):
+            jobs += unit(order[n], order[n - 1] if n else None, sides[n])
+        jobs += [dw_job(1, [(4, 0), (5, 0)], "g"), dzt_job(*order[7]), dw_job(1, [(6, 0), (7, 0)], "g")]
+        last = [dw_job(1, [(i, 1), (i + 1, 1)], "g") for i in range(0, 8, 2)]
+        jobs += last[:3] + weave(dx_jobs(1, 0) + dx_jobs(1, 1), last[3:])
+
+        steps = []
+        for tick in range(len(jobs)):
+            for offset, rank, step in jobs[tick]:
+                steps.append((tick + offset, rank, len(steps), step))
+        for at, rank, n, step in sorted(steps):
+            step()

@@ -24,7 +24,7 @@ EDGE = 1.0 + 3.0 / 256.0
 SMALL_SLOTS = 34
 LARGE_SLOTS = 3
 CODE_SLOTS = 30
-LEAD = 6
+LEAD = 10
 AHEAD = 2
 BEHIND = 3
 
@@ -53,8 +53,8 @@ def tile_gaussian_nn_htanh_v_kernel(
         held = {}
         tiles = {}
 
-        def take(key, kind, shape, dtype):
-            slot = free[kind].pop(0)
+        def take(key, kind, shape, dtype, newest=False):
+            slot = free[kind].pop(-1 if newest else 0)
             held[key] = (kind, slot)
             tag = "%s%d" % (kind, slot)
             if kind == "bank":
@@ -92,18 +92,26 @@ def tile_gaussian_nn_htanh_v_kernel(
                 stop=stop,
             )
 
+        def copy(engine, out, in_):
+            if engine == "s":
+                nc.scalar.copy(out=out, in_=in_)
+            else:
+                nc.vector.tensor_copy(out=out, in_=in_)
+
         def cols(n, width=P):
             return slice(width * n, width * n + width)
 
-        def turn_sum(bank, mean_of, prod_of):
-            for t in range(T):
-                nc.tensor.matmul(bank[:, t, :], lhsT=mean_of(t), rhs=ident_b[:], start=(t == 0), stop=False)
-            for t in range(T):
-                nc.tensor.matmul(bank[:, t, :], lhsT=prod_of(t), rhs=ident_f[:], is_transpose=True, start=False, stop=(t == T - 1))
+        def turn_sum(banks, mean_of, prod_of):
+            for b in range(2):
+                for t in range(T):
+                    nc.tensor.matmul(banks[b][:, t, :], lhsT=mean_of(b, t), rhs=ident_b[:], start=(t == 0), stop=False)
+            for b in range(2):
+                for t in range(T):
+                    nc.tensor.matmul(banks[b][:, t, :], lhsT=prod_of(b, t), rhs=ident_f[:], is_transpose=True, start=False, stop=(t == T - 1))
 
-        READ, QUANT, MAKE, PE, DMA = 1, 2, 3, 0, 4
+        PE, READ, MAKE, QUANT, POOL, DMA = range(6)
 
-        def w2_job(j, q, r):
+        def w2_job(j, q, r, behind=BEHIND, readers="ss"):
             def fetch():
                 if j == 0:
                     load(("sig2", q, r), "small", [P, 2, Y], BF16, sig_W2.rearrange("(a b m) y -> a m b y", b=2, m=P)[2 * q + r])
@@ -130,13 +138,13 @@ def tile_gaussian_nn_htanh_v_kernel(
                     give(("sig2", q, r))
 
             def turn():
-                prod, mu = tiles["prod2", j, q, r], tiles["mean2", q, r]
-                for b in range(2):
-                    bank = take(("w2bank", j, q, r, b), "bank", [P, T, P], F32)
-                    turn_sum(bank, lambda t: mu[:, b, t, :], lambda t: prod[:, b, t, :])
+                prod = tiles["prod2", j, q, r]
+                mean = tiles["mean2", q, r][:] if q == 0 else tiles["mu2", q, r][:].rearrange("p b (w t) -> p b t w", t=T)
+                banks = [take(("w2bank", j, q, r, b), "bank", [P, T, P], F32) for b in range(2)]
+                turn_sum(banks, lambda b, t: mean[:, b, t, :], lambda b, t: prod[:, b, t, :])
                 give(("prod2", j, q, r))
                 if j == J - 1:
-                    give(("mean2", q, r))
+                    give(("mean2" if q == 0 else "mu2", q, r))
 
             def empty():
                 if r == 0:
@@ -145,7 +153,7 @@ def tile_gaussian_nn_htanh_v_kernel(
                 for b in range(2):
                     blocks = cols(2 * r + b, 4)
                     src = tiles["w2bank", j, q, r, b][:].rearrange("p t (b u i) -> p u b i t", u=T, i=8)
-                    nc.scalar.copy(out=dst[:, :, blocks, :, :], in_=src)
+                    copy(readers[b], dst[:, :, blocks, :, :], src)
                     give(("w2bank", j, q, r, b))
 
             def quant():
@@ -153,11 +161,11 @@ def tile_gaussian_nn_htanh_v_kernel(
                 give(("w2in", j, q))
 
             steps = [(-LEAD - AHEAD, DMA, fetch), (-AHEAD, MAKE, multiply), (0, PE, turn), (1, READ, empty)]
-            if j == 0:
+            if j == 0 and q == 0:
                 steps.append((-AHEAD, MAKE, sort_mean))
-            return steps + ([(BEHIND, QUANT, quant)] if r == 1 else [])
+            return steps + ([(behind, QUANT, quant)] if r == 1 else [])
 
-        def grad_job(j, g):
+        def grad_job(j, g, behind=BEHIND):
             def fetch():
                 load(("grad", j, g), "small", [P, T, Y], BF16, grad_out[j].rearrange("(g p t) y -> g p t y", g=2, t=T)[g])
 
@@ -181,30 +189,25 @@ def tile_gaussian_nn_htanh_v_kernel(
                 quantize(("g", j, g), E5M2, ("gin", j, g))
                 give(("gin", j, g))
 
-            return [(-LEAD, DMA, fetch), (0, PE, turn), (1, READ, empty), (BEHIND, QUANT, quant)]
+            return [(-LEAD, DMA, fetch), (0, PE, turn), (1, READ, empty), (behind, QUANT, quant)]
 
         def x_job(g, half, engine):
             def fetch():
-                load(("x", g), "large", [P, T, X], BF16, x.rearrange("(g p t) w -> g p t w", g=2, t=T)[g])
+                load(("x", g, half), "small", [P, T, K], BF16, x.rearrange("(g p t) w -> g p t w", g=2, t=T)[g][:, :, cols(half, K)])
 
             def interleave():
                 dst = take(("xin", g, half), "small", [P, K, T], BF16)
-                src = tiles["x", g][:, :, cols(half, K)].rearrange("p t w -> p w t")
-                if engine == "s":
-                    nc.scalar.copy(out=dst[:], in_=src)
-                else:
-                    nc.vector.tensor_copy(out=dst[:], in_=src)
-                if half == 1:
-                    give(("x", g))
+                src = tiles["x", g, half][:].rearrange("p t w -> p w t")
+                copy(engine, dst[:], src)
+                give(("x", g, half))
 
             def quant():
                 quantize(("xq", g, half), E4M3, ("xin", g, half))
                 give(("xin", g, half))
 
-            steps = [(0, MAKE, interleave), (BEHIND, QUANT, quant)]
-            return steps + ([(-LEAD - AHEAD, DMA, fetch)] if half == 0 else [])
+            return [(-LEAD, DMA, fetch), (0, MAKE, interleave), (2, QUANT, quant)]
 
-        def w1_job(i, j, engine):
+        def w1_job(i, j, pool_ahead=None, readers="ss"):
             a, r = divmod(i, 2)
             xh, c = divmod(i, 4)
             order = "p (b t i) -> p t b i"
@@ -222,8 +225,8 @@ def tile_gaussian_nn_htanh_v_kernel(
                 give(("mu1", a))
 
             def multiply():
-                prod = take(("prod1", i, j), "small", [P, T, 32, 8], F32)
-                eng = nc.gpsimd if engine == "g" else nc.vector
+                prod = take(("prod1", i, j), "small", [P, T, 32, 8], F32, newest=pool_ahead is not None)
+                eng = nc.vector if pool_ahead is None else nc.gpsimd
                 eng.tensor_tensor(
                     out=prod[:],
                     in0=tiles["e1", i][:, j, :].rearrange(order, t=T, i=8),
@@ -236,9 +239,8 @@ def tile_gaussian_nn_htanh_v_kernel(
             def turn():
                 prod = tiles["prod1", i, j][:].rearrange("p t (q b) i -> p t q (b i)", q=2)
                 mean = tiles["mean1", a][:, r].rearrange("p t (q b) i -> p t q (b i)", q=2)
-                for q in range(2):
-                    bank = take(("w1bank", i, j, q), "bank", [P, T, P], F32)
-                    turn_sum(bank, lambda t: mean[:, t, q, :], lambda t: prod[:, t, q, :])
+                banks = [take(("w1bank", i, j, q), "bank", [P, T, P], F32) for q in range(2)]
+                turn_sum(banks, lambda q, t: mean[:, t, q, :], lambda q, t: prod[:, t, q, :])
                 give(("prod1", i, j))
                 if r == 1 and j == J - 1:
                     give(("mean1", a))
@@ -248,14 +250,14 @@ def tile_gaussian_nn_htanh_v_kernel(
                     if c == 0:
                         take(("w1in", j, q, xh), "small", [P, K, T], BF16)
                     src = tiles["w1bank", i, j, q][:].rearrange("p t m -> p m t")
-                    nc.scalar.copy(out=tiles["w1in", j, q, xh][:, cols(c), :], in_=src)
+                    copy(readers[q], tiles["w1in", j, q, xh][:, cols(c), :], src)
                     give(("w1bank", i, j, q))
 
             def quant(q):
                 quantize(("w1", j, q, xh), E4M3, ("w1in", j, q, xh))
                 give(("w1in", j, q, xh))
 
-            steps = [(-AHEAD, MAKE, multiply), (0, PE, turn), (1, READ, empty)]
+            steps = [(-AHEAD, MAKE, multiply) if pool_ahead is None else (-pool_ahead, POOL, multiply), (0, PE, turn), (1, READ, empty)]
             if j == 0:
                 steps.append((-LEAD - AHEAD, DMA, fetch))
                 if r == 0:
@@ -264,7 +266,7 @@ def tile_gaussian_nn_htanh_v_kernel(
                 steps += [(BEHIND, QUANT, lambda: quant(0)), (BEHIND + 1, QUANT, lambda: quant(1))]
             return steps
 
-        def dh_job(j, q, g, half):
+        def dh_job(j, q, g, half, abs_ahead):
             key = (j, q, g)
 
             def fetch():
@@ -273,9 +275,8 @@ def tile_gaussian_nn_htanh_v_kernel(
             def absolute():
                 if half == 0:
                     take(("abs",) + key, "small", [P, K, T], BF16)
-                dst = tiles[("abs",) + key][:].rearrange("p (b v i) t -> p v b i t", v=2, i=16)
-                src = tiles[("z",) + key][:].rearrange("p t (b v i) -> p v b i t", v=2, i=16)
-                nc.scalar.activation(out=dst[:, half], in_=src[:, half], func=ACT.Abs, scale=EDGE)
+                src = tiles[("z",) + key][:, :, cols(half, 256)].rearrange("p t h -> p h t")
+                nc.scalar.activation(out=tiles[("abs",) + key][:, cols(half, 256), :], in_=src, func=ACT.Abs, scale=EDGE)
                 if half == 1:
                     give(("z",) + key)
 
@@ -290,21 +291,22 @@ def tile_gaussian_nn_htanh_v_kernel(
                     give(("w2", j, q))
 
             def mask():
-                if half == 0:
-                    take(("dz",) + key, "small", [P, K, T], BF16)
+                take(("dz",) + key, "small", [P, K, T], BF16)
                 size = tiles[("abs",) + key][:].rearrange("p (b u i) t -> p u b i t", u=T, i=8)
                 dz = tiles[("dz",) + key][:].rearrange("p (u b i) t -> p u b i t", u=T, i=8)
-                for u in (2 * half, 2 * half + 1):
+                for u in range(T):
                     bank = tiles[("dh",) + key + (u,)][:].rearrange("p t (b i) -> p b i t", i=8)
                     nc.vector.scalar_tensor_tensor(out=dz[:, u], in0=size[:, u], scalar=EDGE, in1=bank, op0=ALU.is_lt, op1=ALU.mult)
                     give(("dh",) + key + (u,))
-                if half == 1:
-                    give(("abs",) + key)
+                give(("abs",) + key)
 
-            steps = [(-AHEAD, MAKE, absolute), (0, PE, multiply), (1, READ, mask)]
+            def quant_tokens():
+                quantize(("dzn",) + key, E5M2, ("dz",) + key)
+
+            steps = [(-abs_ahead, MAKE, absolute), (0, PE, multiply)]
             if half == 0:
-                steps += [(-LEAD - AHEAD, DMA, fetch)]
-            return steps
+                return steps + [(-LEAD - abs_ahead, DMA, fetch)]
+            return steps + [(1, READ, mask), (2, QUANT, quant_tokens)]
 
         def dzt_job(j, q, g):
             key = (j, q, g)
@@ -317,9 +319,6 @@ def tile_gaussian_nn_htanh_v_kernel(
                         nc.tensor.transpose(bank[:, u, :], words[:, u, :, s], ident_f[:])
                 give(("dz",) + key)
 
-            def quant_tokens():
-                quantize(("dzn",) + key, E5M2, ("dz",) + key)
-
             def empty():
                 dst = take(("dzin",) + key, "small", [P, K, T], BF16)
                 for s in range(2):
@@ -331,15 +330,17 @@ def tile_gaussian_nn_htanh_v_kernel(
                 quantize(("dzh",) + key, E5M2, ("dzin",) + key)
                 give(("dzin",) + key)
 
-            return [(0, PE, turn), (-1, QUANT, quant_tokens), (1, READ, empty), (BEHIND, QUANT, quant_features)]
+            return [(0, PE, turn), (1, READ, empty), (BEHIND, QUANT, quant_features)]
 
-        def dx_job(g, xh, t):
-            pair = (g, xh, t // 2)
+        def dx_job(g, xh, t, width=2, passes=range(4)):
+            pair = (g, xh, t // width)
 
             def multiply():
-                bank = take(("dx", g, xh, t), "bank", [P, K], F32)
-                for k in range(4):
-                    j, q = divmod(k, 2)
+                if 0 in passes:
+                    take(("dx", g, xh, t), "bank", [P, K], F32)
+                bank = tiles["dx", g, xh, t]
+                for k in passes:
+                    q, j = divmod(k, 2)
                     mx(bank[:], ("dzh", j, q, g), cols(t), E5M2, ("w1", j, q, xh), cols(0, K), E4M3, k == 0, k == 3)
                     if t == T - 1 and xh == 1:
                         give(("dzh", j, q, g))
@@ -347,17 +348,19 @@ def tile_gaussian_nn_htanh_v_kernel(
                         give(("w1", j, q, xh))
 
             def empty():
-                if t % 2 == 0:
-                    take(("out0",) + pair, "small", [P, 2, K], F32)
-                nc.scalar.copy(out=tiles[("out0",) + pair][:, t % 2, :], in_=tiles["dx", g, xh, t][:])
+                if t % width == 0:
+                    take(("out0",) + pair, "small", [P, width, K], F32)
+                nc.scalar.copy(out=tiles[("out0",) + pair][:, t % width, :], in_=tiles["dx", g, xh, t][:])
                 give(("dx", g, xh, t))
 
             def store():
-                dst = out_0.rearrange("(g p t) w -> g p t w", g=2, t=T)[g][:, cols(t // 2, 2), cols(xh, K)]
+                dst = out_0.rearrange("(g p t) w -> g p t w", g=2, t=T)[g][:, cols(t // width, width), cols(xh, K)]
                 nc.sync.dma_start(out=dst, in_=tiles[("out0",) + pair][:])
                 give(("out0",) + pair)
 
-            return [(0, PE, multiply), (1, READ, empty)] + ([(1, DMA, store)] if t % 2 == 1 else [])
+            if 3 not in passes:
+                return [(0, PE, multiply)]
+            return [(0, PE, multiply), (1, READ, empty)] + ([(1, DMA, store)] if t % width == width - 1 else [])
 
         def dw_job(q, items, engine):
             def multiply():
@@ -384,7 +387,7 @@ def tile_gaussian_nn_htanh_v_kernel(
 
             def add(i):
                 first, second = tiles["part", q, i // 2, 0][:, i % 2, :], tiles["part", q, i // 2, 1][:, i % 2, :]
-                eng = nc.gpsimd if engine == "g" else nc.vector
+                eng = nc.gpsimd if engine[i % len(engine)] == "g" else nc.vector
                 eng.tensor_tensor(out=first, in0=first, in1=second, op=ALU.add)
                 if i % 2 == 1:
                     give(("part", q, i // 2, 1))
@@ -402,15 +405,21 @@ def tile_gaussian_nn_htanh_v_kernel(
             return [w2_job(j, q, r) for r in range(2)]
 
         def w1_jobs(rows):
-            return [w1_job(i, j, "v") for i in rows for j in range(J)]
+            return [w1_job(i, j) for i in rows for j in range(J)]
 
-        def dx_jobs(g, xh):
-            return [dx_job(g, xh, t) for t in range(T)]
+        def dx_jobs(g, xh, width=2, passes=range(4)):
+            return [dx_job(g, xh, t, width, passes) for t in range(T)]
 
-        def unit(key, last, side):
-            turn = [dzt_job(*last)] if last else []
-            n = len(side) // 2
-            return [dh_job(*key, 0)] + side[:1] + turn + side[1:n] + [dh_job(*key, 1)] + side[n:]
+        def dw_jobs(q, j, engine):
+            return [dw_job(q, [(i, j), (i + 1, j)], engine) for i in range(0, 8, 2)]
+
+        jobs = []
+        starts = []
+
+        def unit(key, early, late):
+            ahead = len(jobs) - starts[-1] - 1 if starts else 2
+            starts.append(len(jobs))
+            jobs.extend([dh_job(*key, 0, ahead), dh_job(*key, 1, ahead)] + early + [dzt_job(*key)] + late)
 
         def weave(first, second):
             jobs = []
@@ -421,22 +430,24 @@ def tile_gaussian_nn_htanh_v_kernel(
         order = [(j, q, g) for g in range(2) for q in range(2) for j in range(J)]
         first = dx_jobs(0, 0) + dx_jobs(0, 1)
         first = dx_jobs(0, 0) + dx_jobs(0, 1)
-        sides = [
-            w2_jobs(0, 1) + w2_jobs(1, 1),
-            w1_jobs([0, 1]),
-            w1_jobs([2, 3]),
-            [grad_job(0, 1)] + w1_jobs([4, 5]),
-            [grad_job(1, 1)] + w1_jobs([6, 7]) + [x_job(0, 0, "v")],
-            weave([x_job(0, 1, "s"), x_job(1, 0, "v"), x_job(1, 1, "v")], first[:6]),
-            first[6:7] + [dw_job(0, [(i, 0), (i, 1)], "g") for i in range(7)],
-            first[7:] + [dw_job(0, [(7, 0), (7, 1)], "g")] + [dw_job(1, [(i, 0), (i + 1, 0)], "g") for i in range(0, 4, 2)],
-        ]
-        jobs = w2_jobs(0, 0) + [grad_job(0, 0)] + w2_jobs(1, 0) + [grad_job(1, 0)]
-        for n in range(8):
-            jobs += unit(order[n], order[n - 1] if n else None, sides[n])
-        jobs += [dw_job(1, [(4, 0), (5, 0)], "g"), dzt_job(*order[7]), dw_job(1, [(6, 0), (7, 0)], "g")]
-        last = [dw_job(1, [(i, 1), (i + 1, 1)], "g") for i in range(0, 8, 2)]
-        jobs += last[:3] + weave(dx_jobs(1, 0) + dx_jobs(1, 1), last[3:])
+        def w1(n, pool_ahead=None, readers="ss"):
+            return w1_job(n // 2, n % 2, pool_ahead, readers)
+
+        jobs.extend([w2_job(0, 0, 0), w2_job(0, 0, 1, 2), grad_job(0, 0, 2), w2_job(1, 0, 0, readers="vv"), w2_job(1, 0, 1, readers="sv")])
+        unit(order[0], [grad_job(1, 0)] + w2_jobs(0, 1), w2_jobs(1, 1))
+        unit(order[1], [w1(0, None, "vs"), w1(1), w1(2, 3)], [w1(3)])
+        unit(order[2], [w1(4, None, "vs"), w1(5), w1(6, 3)], [w1(7)])
+        unit(order[3], [w1(8, None, "vs"), grad_job(0, 1), w1(9, 3)], [w1(10), w1(11), grad_job(1, 1)])
+        dx = dx_jobs(0, 0)
+        unit(order[4], [dx[0], dx[1] + x_job(0, 0, "v"), w1(12, 3), w1(13)], [w1(14), w1(15) + x_job(0, 1, "v"), dx[2], dx[3]])
+        dx = dx_jobs(0, 1)
+        dw = dw_jobs(0, 0, "g")
+        unit(order[5], [x_job(1, 0, "s") + dx[0], x_job(1, 1, "v") + dx[1], dx[2]], [dx[3]] + dw)
+        unit(order[6], dw_jobs(0, 1, "g")[:3], dw_jobs(0, 1, "g")[3:] + dw_jobs(1, 0, "g"))
+        early = dx_jobs(1, 0, 2, range(3))
+        unit(order[7], [[], early[0] + early[1], early[2] + early[3]], dw_jobs(1, 1, "vg")[:3])
+        late = dx_jobs(1, 0, 2, [3])
+        jobs.extend([late[0] + late[1], late[2] + late[3]] + weave(dw_jobs(1, 1, "vg")[3:], dx_jobs(1, 1, 1)))
 
         steps = []
         for tick in range(len(jobs)):

@@ -1,4 +1,5 @@
 from contextlib import ExitStack
+from functools import partial
 
 import concourse.mybir as mybir
 from concourse.masks import make_identity
@@ -9,6 +10,7 @@ F32 = mybir.dt.float32
 BF16 = mybir.dt.bfloat16
 U32 = mybir.dt.uint32
 U8 = mybir.dt.uint8
+I32 = mybir.dt.int32
 E4M3 = mybir.dt.float8_e4m3fn_x4
 E5M2 = mybir.dt.float8_e5m2_x4
 ALU = mybir.AluOpType
@@ -21,6 +23,7 @@ P = 128
 T = 4
 K = 512
 EDGE = 1.0 + 3.0 / 256.0
+CENTRE = 3.0 * 2.0**22 + 1.0
 SMALL_SLOTS = 34
 LARGE_SLOTS = 3
 CODE_SLOTS = 30
@@ -75,12 +78,25 @@ def tile_gaussian_nn_htanh_v_kernel(
         def load(key, kind, shape, dtype, src):
             nc.sync.dma_start(out=take(key, kind, shape, dtype)[:], in_=src)
 
-        def quantize(key, fmt, src_key):
+        sources = {}
+
+        def quantize(key):
+            if key in tiles:
+                return
+            fmt, src_key, last_reader = sources[key]
             words, scales = take(key, "code", [P, K], U32)
             src = tiles[src_key][:].rearrange("p c t -> p (c t)")
             nc.vector.quantize_mx(out=words[:].bitcast(fmt), scales=scales[:], in_=src)
+            if last_reader:
+                give(src_key)
+
+        def quant_step(offset, key, fmt, src_key, last_reader=True):
+            sources[key] = (fmt, src_key, last_reader)
+            return (offset, QUANT, partial(quantize, key))
 
         def mx(bank, lhs_key, lhs_cols, lhs_fmt, rhs_key, rhs_cols, rhs_fmt, start, stop):
+            quantize(lhs_key)
+            quantize(rhs_key)
             lhs, rhs = tiles[lhs_key], tiles[rhs_key]
             nc.tensor.matmul_mx(
                 out=bank,
@@ -95,56 +111,72 @@ def tile_gaussian_nn_htanh_v_kernel(
         def copy(engine, out, in_):
             if engine == "s":
                 nc.scalar.copy(out=out, in_=in_)
+            elif engine == "g":
+                nc.gpsimd.tensor_scalar(out=out, in0=in_, scalar1=1.0, scalar2=0.0, op0=ALU.mult, op1=ALU.add)
             else:
                 nc.vector.tensor_copy(out=out, in_=in_)
 
         def cols(n, width=P):
             return slice(width * n, width * n + width)
 
-        def turn_sum(banks, mean_of, prod_of):
-            for b in range(2):
-                for t in range(T):
-                    nc.tensor.matmul(banks[b][:, t, :], lhsT=mean_of(b, t), rhs=ident_b[:], start=(t == 0), stop=False)
-            for b in range(2):
-                for t in range(T):
-                    nc.tensor.matmul(banks[b][:, t, :], lhsT=prod_of(b, t), rhs=ident_f[:], is_transpose=True, start=False, stop=(t == T - 1))
+        def turn_sum(banks, mean_of, prod_of, mean_first):
+            for second in (False, True):
+                for b in range(2):
+                    for t in range(T):
+                        flags = dict(start=(t == 0 and not second), stop=(t == T - 1 and second))
+                        if mean_first != second:
+                            nc.tensor.matmul(banks[b][:, t, :], lhsT=mean_of(b, t), rhs=ident_b[:], **flags)
+                        else:
+                            nc.tensor.matmul(banks[b][:, t, :], lhsT=prod_of(b, t), rhs=ident_f[:], is_transpose=True, **flags)
 
         PE, READ, MAKE, QUANT, POOL, DMA = range(6)
 
-        def w2_job(j, q, r, behind=BEHIND, readers="ss"):
+        def w2_job(j, q, r, mean_first, behind=BEHIND, readers="ss"):
+            split = j == 0 and q == 0
+            part = r if split else 0
+
+            def rows(key):
+                return tiles[key + (part,)][:, cols(0 if split else r, 2), :]
+
             def fetch():
-                if j == 0:
-                    load(("sig2", q, r), "small", [P, 2, Y], BF16, sig_W2.rearrange("(a b m) y -> a m b y", b=2, m=P)[2 * q + r])
-                load(("e2", j, q, r), "small", [P, 2, Y], BF16, e_W2[j].rearrange("(a b m) y -> a m b y", b=2, m=P)[2 * q + r])
-                if j == 0:
-                    load(("mu2", q, r), "small", [P, 2, Y], BF16, mu_W2.rearrange("(a b m) y -> a m b y", b=2, m=P)[2 * q + r])
+                wanted = [(("sig2", q), sig_W2), (("e2", j, q), e_W2[j]), (("mu2", q), mu_W2)]
+                for key, src in wanted if j == 0 else wanted[1:2]:
+                    blocks = 2 if split else 4
+                    view = src.rearrange("(a b m) y -> a m b y", b=blocks, m=P)[2 * q + r if split else q]
+                    load(key + (part,), "small", [P, blocks, Y], BF16, view)
+
+            def shared(name):
+                return tiles[name, q, r][:] if q == 0 else tiles[name, q, 0][:, cols(r, 2), :]
+
+            def release(name):
+                if j == J - 1 and (q == 0 or r == 1):
+                    give((name, q, r if q == 0 else 0))
 
             def sort_mean():
                 dst = take(("mean2", q, r), "small", [P, 2, T, P], BF16)
-                nc.scalar.copy(out=dst[:], in_=tiles["mu2", q, r][:].rearrange("p b (w t) -> p b t w", t=T))
+                copy("s", dst[:], shared("mu2").rearrange("p b (w t) -> p b t w", t=T))
                 give(("mu2", q, r))
 
             def multiply():
                 prod = take(("prod2", j, q, r), "small", [P, 2, T, P], F32)
                 order = "p b (w t) -> p b t w"
                 nc.vector.tensor_tensor(
-                    out=prod[:],
-                    in0=tiles["e2", j, q, r][:].rearrange(order, t=T),
-                    in1=tiles["sig2", q, r][:].rearrange(order, t=T),
-                    op=ALU.mult,
+                    out=prod[:], in0=rows(("e2", j, q)).rearrange(order, t=T), in1=shared("sig2").rearrange(order, t=T), op=ALU.mult
                 )
-                give(("e2", j, q, r))
-                if j == J - 1:
-                    give(("sig2", q, r))
+                if split or r == 1:
+                    give(("e2", j, q, part))
+                release("sig2")
 
             def turn():
                 prod = tiles["prod2", j, q, r]
-                mean = tiles["mean2", q, r][:] if q == 0 else tiles["mu2", q, r][:].rearrange("p b (w t) -> p b t w", t=T)
+                mean = tiles["mean2", q, r] if q == 0 else shared("mu2").rearrange("p b (w t) -> p b t w", t=T)
                 banks = [take(("w2bank", j, q, r, b), "bank", [P, T, P], F32) for b in range(2)]
-                turn_sum(banks, lambda b, t: mean[:, b, t, :], lambda b, t: prod[:, b, t, :])
+                turn_sum(banks, lambda b, t: mean[:, b, t, :], lambda b, t: prod[:, b, t, :], mean_first)
                 give(("prod2", j, q, r))
-                if j == J - 1:
-                    give(("mean2" if q == 0 else "mu2", q, r))
+                if j == J - 1 and q == 0:
+                    give(("mean2", q, r))
+                if q == 1:
+                    release("mu2")
 
             def empty():
                 if r == 0:
@@ -156,16 +188,14 @@ def tile_gaussian_nn_htanh_v_kernel(
                     copy(readers[b], dst[:, :, blocks, :, :], src)
                     give(("w2bank", j, q, r, b))
 
-            def quant():
-                quantize(("w2", j, q), E4M3, ("w2in", j, q))
-                give(("w2in", j, q))
-
-            steps = [(-LEAD - AHEAD, DMA, fetch), (-AHEAD, MAKE, multiply), (0, PE, turn), (1, READ, empty)]
-            if j == 0 and q == 0:
+            steps = [(-AHEAD, MAKE, multiply), (0, PE, turn), (1, READ, empty)]
+            if split or r == 0:
+                steps.append((-LEAD - AHEAD, DMA, fetch))
+            if split:
                 steps.append((-AHEAD, MAKE, sort_mean))
-            return steps + ([(behind, QUANT, quant)] if r == 1 else [])
+            return steps + ([quant_step(behind, ("w2", j, q), E4M3, ("w2in", j, q))] if r == 1 else [])
 
-        def grad_job(j, g, behind=BEHIND):
+        def grad_job(j, g, behind=BEHIND, readers="ss"):
             def fetch():
                 load(("grad", j, g), "small", [P, T, Y], BF16, grad_out[j].rearrange("(g p t) y -> g p t y", g=2, t=T)[g])
 
@@ -182,32 +212,30 @@ def tile_gaussian_nn_htanh_v_kernel(
                 dst = take(("gin", j, g), "small", [P, K, T], BF16)[:].rearrange("p c t -> p (c t)").bitcast(F32)
                 for a in range(2):
                     out = dst[:, cols(a, K)].rearrange("p (s m u) -> p s m u", s=2, u=2)
-                    nc.scalar.copy(out=out, in_=tiles["gbank", j, g, a][:].rearrange("p s u m -> p s m u"))
+                    copy(readers[a], out, tiles["gbank", j, g, a][:].rearrange("p s u m -> p s m u"))
                     give(("gbank", j, g, a))
 
-            def quant():
-                quantize(("g", j, g), E5M2, ("gin", j, g))
-                give(("gin", j, g))
+            return [(-LEAD, DMA, fetch), (0, PE, turn), (1, READ, empty), quant_step(behind, ("g", j, g), E5M2, ("gin", j, g))]
 
-            return [(-LEAD, DMA, fetch), (0, PE, turn), (1, READ, empty), (behind, QUANT, quant)]
-
-        def x_job(g, half, engine):
+        def x_job(g, half, engines, behind=3):
             def fetch():
                 load(("x", g, half), "small", [P, T, K], BF16, x.rearrange("(g p t) w -> g p t w", g=2, t=T)[g][:, :, cols(half, K)])
 
-            def interleave():
-                dst = take(("xin", g, half), "small", [P, K, T], BF16)
-                src = tiles["x", g, half][:].rearrange("p t w -> p w t")
-                copy(engine, dst[:], src)
-                give(("x", g, half))
+            def interleave(n):
+                if n == 0:
+                    take(("xin", g, half), "small", [P, K, T], BF16, newest=engines == "gg")
+                src = tiles["x", g, half][:, :, cols(n, 256)].rearrange("p t w -> p w t")
+                copy(engines[n], tiles["xin", g, half][:, cols(n, 256), :], src)
+                if n == 1:
+                    give(("x", g, half))
 
-            def quant():
-                quantize(("xq", g, half), E4M3, ("xin", g, half))
-                give(("xin", g, half))
+            if engines == "gg":
+                steps = [(0, POOL, partial(interleave, n)) for n in range(2)]
+            else:
+                steps = [(n, MAKE, partial(interleave, n)) for n in range(2)]
+            return steps + [(-LEAD, DMA, fetch), quant_step(behind, ("xq", g, half), E4M3, ("xin", g, half))]
 
-            return [(-LEAD, DMA, fetch), (0, MAKE, interleave), (2, QUANT, quant)]
-
-        def w1_job(i, j, pool_ahead=None, readers="ss"):
+        def w1_job(i, j, mean_first, pool_ahead=None, readers="ss", sorter="v", behind=BEHIND, ahead=AHEAD):
             a, r = divmod(i, 2)
             xh, c = divmod(i, 4)
             order = "p (b t i) -> p t b i"
@@ -221,7 +249,7 @@ def tile_gaussian_nn_htanh_v_kernel(
 
             def sort_mean():
                 dst = take(("mean1", a), "small", [P, 2, T, 32, 8], BF16)
-                nc.vector.tensor_copy(out=dst[:], in_=tiles["mu1", a][:].rearrange("p r (b t i) -> p r t b i", t=T, i=8))
+                copy(sorter, dst[:], tiles["mu1", a][:].rearrange("p r (b t i) -> p r t b i", t=T, i=8))
                 give(("mu1", a))
 
             def multiply():
@@ -240,7 +268,7 @@ def tile_gaussian_nn_htanh_v_kernel(
                 prod = tiles["prod1", i, j][:].rearrange("p t (q b) i -> p t q (b i)", q=2)
                 mean = tiles["mean1", a][:, r].rearrange("p t (q b) i -> p t q (b i)", q=2)
                 banks = [take(("w1bank", i, j, q), "bank", [P, T, P], F32) for q in range(2)]
-                turn_sum(banks, lambda q, t: mean[:, t, q, :], lambda q, t: prod[:, t, q, :])
+                turn_sum(banks, lambda q, t: mean[:, t, q, :], lambda q, t: prod[:, t, q, :], mean_first)
                 give(("prod1", i, j))
                 if r == 1 and j == J - 1:
                     give(("mean1", a))
@@ -253,31 +281,31 @@ def tile_gaussian_nn_htanh_v_kernel(
                     copy(readers[q], tiles["w1in", j, q, xh][:, cols(c), :], src)
                     give(("w1bank", i, j, q))
 
-            def quant(q):
-                quantize(("w1", j, q, xh), E4M3, ("w1in", j, q, xh))
-                give(("w1in", j, q, xh))
-
-            steps = [(-AHEAD, MAKE, multiply) if pool_ahead is None else (-pool_ahead, POOL, multiply), (0, PE, turn), (1, READ, empty)]
+            steps = [(-ahead, MAKE, multiply) if pool_ahead is None else (-pool_ahead, POOL, multiply), (0, PE, turn), (1, READ, empty)]
             if j == 0:
                 steps.append((-LEAD - AHEAD, DMA, fetch))
                 if r == 0:
                     steps.append((-AHEAD - 1, MAKE, sort_mean))
             if c == 3:
-                steps += [(BEHIND, QUANT, lambda: quant(0)), (BEHIND + 1, QUANT, lambda: quant(1))]
+                steps += [quant_step(behind + q, ("w1", j, q, xh), E4M3, ("w1in", j, q, xh)) for q in range(2)]
             return steps
 
-        def dh_job(j, q, g, half, abs_ahead):
+        def dh_job(j, q, g, half, abs_ahead, markers):
             key = (j, q, g)
+            pieces = [(0, 2), (2, 2)] if markers[2] == markers[3] else [(0, 2), (2, 1), (3, 1)]
 
             def fetch():
                 load(("z",) + key, "large", [P, T, K], F32, z1[j].rearrange("(g p t) h -> g p t h", g=2, t=T)[g][:, :, cols(q, K)])
 
-            def absolute():
-                if half == 0:
-                    take(("abs",) + key, "small", [P, K, T], BF16)
-                src = tiles[("z",) + key][:, :, cols(half, 256)].rearrange("p t h -> p h t")
-                nc.scalar.activation(out=tiles[("abs",) + key][:, cols(half, 256), :], in_=src, func=ACT.Abs, scale=EDGE)
-                if half == 1:
+            def mark(u, n):
+                src = tiles[("z",) + key][:].rearrange("p t (b h) -> p b h t", h=32)[:, :, 8 * u : 8 * (u + n), :]
+                if markers[u] == "s":
+                    dst = take(("mark",) + key + (u,), "small", [P, 16, 8 * n, T], BF16)
+                    nc.scalar.activation(out=dst[:], in_=src, func=ACT.Abs, scale=EDGE)
+                else:
+                    dst = take(("mark",) + key + (u,), "small", [P, 16, 8 * n, T], I32, newest=(u == 0))
+                    nc.gpsimd.tensor_scalar(out=dst[:], in0=src, scalar1=0.5, scalar2=CENTRE, op0=ALU.mult, op1=ALU.add)
+                if u + n == T:
                     give(("z",) + key)
 
             def multiply():
@@ -292,23 +320,27 @@ def tile_gaussian_nn_htanh_v_kernel(
 
             def mask():
                 take(("dz",) + key, "small", [P, K, T], BF16)
-                size = tiles[("abs",) + key][:].rearrange("p (b u i) t -> p u b i t", u=T, i=8)
                 dz = tiles[("dz",) + key][:].rearrange("p (u b i) t -> p u b i t", u=T, i=8)
                 for u in range(T):
                     bank = tiles[("dh",) + key + (u,)][:].rearrange("p t (b i) -> p b i t", i=8)
-                    nc.vector.scalar_tensor_tensor(out=dz[:, u], in0=size[:, u], scalar=EDGE, in1=bank, op0=ALU.is_lt, op1=ALU.mult)
+                    first, n = [piece for piece in pieces if piece[0] <= u][-1]
+                    marks = tiles[("mark",) + key + (first,)][:, :, cols(u - first, 8), :]
+                    level, test = (EDGE, ALU.is_lt) if markers[u] == "s" else (CENTRE, ALU.is_equal)
+                    nc.vector.scalar_tensor_tensor(out=dz[:, u], in0=marks, scalar=level, in1=bank, op0=test, op1=ALU.mult)
                     give(("dh",) + key + (u,))
-                give(("abs",) + key)
+                    if u == first + n - 1:
+                        give(("mark",) + key + (first,))
 
-            def quant_tokens():
-                quantize(("dzn",) + key, E5M2, ("dz",) + key)
-
-            steps = [(-abs_ahead, MAKE, absolute), (0, PE, multiply)]
+            steps = [(0, PE, multiply)]
             if half == 0:
-                return steps + [(-LEAD - abs_ahead, DMA, fetch)]
-            return steps + [(1, READ, mask), (2, QUANT, quant_tokens)]
+                steps.append((-LEAD - abs_ahead, DMA, fetch))
+                for u, n in pieces:
+                    at = (-abs_ahead, POOL) if markers[u] == "g" else (-abs_ahead + 1 + u // 2, MAKE)
+                    steps.append(at + (partial(mark, u, n),))
+                return steps
+            return steps + [(1, READ, mask), quant_step(2, ("dzn",) + key, E5M2, ("dz",) + key, False)]
 
-        def dzt_job(j, q, g):
+        def dzt_job(j, q, g, behind):
             key = (j, q, g)
 
             def turn():
@@ -326,13 +358,9 @@ def tile_gaussian_nn_htanh_v_kernel(
                     nc.scalar.copy(out=dst[:, cols(s, 256), :].rearrange("p (e m) u -> p e m u", e=2), in_=src)
                     give(("dzbank",) + key + (s,))
 
-            def quant_features():
-                quantize(("dzh",) + key, E5M2, ("dzin",) + key)
-                give(("dzin",) + key)
+            return [(0, PE, turn), (1, READ, empty), quant_step(behind, ("dzh",) + key, E5M2, ("dzin",) + key)]
 
-            return [(0, PE, turn), (1, READ, empty), (BEHIND, QUANT, quant_features)]
-
-        def dx_job(g, xh, t, width=2, passes=range(4)):
+        def dx_job(g, xh, t, width=2, passes=range(4), reader="s"):
             pair = (g, xh, t // width)
 
             def multiply():
@@ -350,7 +378,7 @@ def tile_gaussian_nn_htanh_v_kernel(
             def empty():
                 if t % width == 0:
                     take(("out0",) + pair, "small", [P, width, K], F32)
-                nc.scalar.copy(out=tiles[("out0",) + pair][:, t % width, :], in_=tiles["dx", g, xh, t][:])
+                copy(reader, tiles[("out0",) + pair][:, t % width, :], tiles["dx", g, xh, t][:])
                 give(("dx", g, xh, t))
 
             def store():
@@ -362,7 +390,7 @@ def tile_gaussian_nn_htanh_v_kernel(
                 return [(0, PE, multiply)]
             return [(0, PE, multiply), (1, READ, empty)] + ([(1, DMA, store)] if t % width == width - 1 else [])
 
-        def dw_job(q, items, engine):
+        def dw_job(q, items, engine, store_behind=1):
             def multiply():
                 for i, j in items:
                     bank = take(("dw", q, i, j), "bank", [P, K], F32)
@@ -399,13 +427,7 @@ def tile_gaussian_nn_htanh_v_kernel(
 
             done = [i for i, j in items if j == J - 1]
             steps = [(0, PE, multiply), (1, READ, weigh), (1, MAKE, lambda: [add(i) for i in done])]
-            return steps + [(1, DMA, lambda: [store(i) for i in done if i % 2 == 1])]
-
-        def w2_jobs(j, q):
-            return [w2_job(j, q, r) for r in range(2)]
-
-        def w1_jobs(rows):
-            return [w1_job(i, j) for i in rows for j in range(J)]
+            return steps + [(store_behind, DMA, lambda: [store(i) for i in done if i % 2 == 1])]
 
         def dx_jobs(g, xh, width=2, passes=range(4)):
             return [dx_job(g, xh, t, width, passes) for t in range(T)]
@@ -416,10 +438,10 @@ def tile_gaussian_nn_htanh_v_kernel(
         jobs = []
         starts = []
 
-        def unit(key, early, late):
+        def unit(key, markers, early, late, behind=BEHIND, beside=()):
             ahead = len(jobs) - starts[-1] - 1 if starts else 2
             starts.append(len(jobs))
-            jobs.extend([dh_job(*key, 0, ahead), dh_job(*key, 1, ahead)] + early + [dzt_job(*key)] + late)
+            jobs.extend([dh_job(*key, 0, ahead, markers), dh_job(*key, 1, ahead, markers) + list(beside)] + early + [dzt_job(*key, behind)] + late)
 
         def weave(first, second):
             jobs = []
@@ -430,24 +452,25 @@ def tile_gaussian_nn_htanh_v_kernel(
         order = [(j, q, g) for g in range(2) for q in range(2) for j in range(J)]
         first = dx_jobs(0, 0) + dx_jobs(0, 1)
         first = dx_jobs(0, 0) + dx_jobs(0, 1)
-        def w1(n, pool_ahead=None, readers="ss"):
-            return w1_job(n // 2, n % 2, pool_ahead, readers)
+        def w1(n, mean_first, pool_ahead=None, readers="ss", behind=BEHIND, ahead=3, sorter="v"):
+            return w1_job(n // 2, n % 2, mean_first, pool_ahead, readers, sorter, behind, ahead)
 
-        jobs.extend([w2_job(0, 0, 0), w2_job(0, 0, 1, 2), grad_job(0, 0, 2), w2_job(1, 0, 0, readers="vv"), w2_job(1, 0, 1, readers="sv")])
-        unit(order[0], [grad_job(1, 0)] + w2_jobs(0, 1), w2_jobs(1, 1))
-        unit(order[1], [w1(0, None, "vs"), w1(1), w1(2, 3)], [w1(3)])
-        unit(order[2], [w1(4, None, "vs"), w1(5), w1(6, 3)], [w1(7)])
-        unit(order[3], [w1(8, None, "vs"), grad_job(0, 1), w1(9, 3)], [w1(10), w1(11), grad_job(1, 1)])
+        jobs.extend([w2_job(0, 0, 0, False), w2_job(0, 0, 1, True, 2), grad_job(0, 0, 1, "vv"), w2_job(1, 0, 0, False)])
+        unit(order[0], "ssss", [w2_job(1, 0, 1, True), grad_job(1, 0)], [w2_job(0, 1, 0, False), w2_job(0, 1, 1, True), w2_job(1, 1, 0, False)], 5)
+        unit(order[1], "gggg", [w2_job(1, 1, 1, True), w1(0, False), w1(1, True, 3)], [w1(2, False)], 3)
+        unit(order[2], "ssss", [w1(3, True), w1(4, False), w1(5, True, 3, "vs")], [w1(6, False), w1(7, False)], 4)
+        unit(order[3], "ssss", [w1(8, True), grad_job(0, 1, 4), w1(9, True)], [w1(10, False) + x_job(0, 1, "vv"), w1(11, True), grad_job(1, 1, 5)], 5, x_job(0, 0, "gg", 5))
         dx = dx_jobs(0, 0)
-        unit(order[4], [dx[0], dx[1] + x_job(0, 0, "v"), w1(12, 3), w1(13)], [w1(14), w1(15) + x_job(0, 1, "v"), dx[2], dx[3]])
-        dx = dx_jobs(0, 1)
+        unit(order[4], "ssss", [dx[0], dx[1], w1(12, True)], [w1(13, False), dx[2] + x_job(1, 1, "vv", 3), dx[3]], 5, x_job(1, 0, "gg", 5))
         dw = dw_jobs(0, 0, "g")
-        unit(order[5], [x_job(1, 0, "s") + dx[0], x_job(1, 1, "v") + dx[1], dx[2]], [dx[3]] + dw)
-        unit(order[6], dw_jobs(0, 1, "g")[:3], dw_jobs(0, 1, "g")[3:] + dw_jobs(1, 0, "g"))
-        early = dx_jobs(1, 0, 2, range(3))
-        unit(order[7], [[], early[0] + early[1], early[2] + early[3]], dw_jobs(1, 1, "vg")[:3])
-        late = dx_jobs(1, 0, 2, [3])
-        jobs.extend([late[0] + late[1], late[2] + late[3]] + weave(dw_jobs(1, 1, "vg")[3:], dx_jobs(1, 1, 1)))
+        unit(order[5], "ssss", [dw[0], dw[1], w1(14, True, 3)], [w1(15, False, 3), dw[2], dw[3]], 5)
+        dx = dx_jobs(0, 1)
+        dw = dw_jobs(0, 1, "g")
+        unit(order[6], "ssss", dw[:2] + dx[:1], weave(dw[2:], dx[1:]), 3)
+        both = [(i, 0) for i in range(4)] + [(i, 1) for i in range(4)] + [(i, j) for i in range(4, 8) for j in range(J)]
+        dw = [dw_job(1, both[n : n + 2], "vgvggggg", 3) for n in range(0, 16, 2)]
+        unit(order[7], "ssss", dw[:2], dw[2:5], 2)
+        jobs.extend(weave(dx_jobs(1, 0) + dx_jobs(1, 1, 1), dw[5:]))
 
         steps = []
         for tick in range(len(jobs)):

@@ -30,6 +30,8 @@ CODE_SLOTS = 30
 LEAD = 10
 AHEAD = 2
 BEHIND = 3
+SORTED = 1
+WARM = 0
 
 
 def tile_gaussian_nn_htanh_v_kernel(
@@ -131,7 +133,7 @@ def tile_gaussian_nn_htanh_v_kernel(
 
         PE, READ, MAKE, QUANT, POOL, DMA = range(6)
 
-        def w2_job(j, q, r, mean_first, behind=BEHIND, readers="ss"):
+        def w2_job(j, q, r, mean_first, behind=BEHIND, readers="ss", sorter="s", ahead=AHEAD):
             split = j == 0 and q == 0
             part = r if split else 0
 
@@ -152,10 +154,19 @@ def tile_gaussian_nn_htanh_v_kernel(
                 if j == J - 1 and (q == 0 or r == 1):
                     give((name, q, r if q == 0 else 0))
 
+            def warm_up():
+                for n in range(WARM):
+                    if n == 0:
+                        bank = take(("warm",), "bank", [P, K], F32)
+                    nc.tensor.matmul(tiles["warm",][:], lhsT=ident_b[:], rhs=shared("sig2")[:, 0, :], start=True, stop=True)
+                if WARM:
+                    give(("warm",))
+
             def sort_mean():
                 dst = take(("mean2", q, r), "small", [P, 2, T, P], BF16)
-                copy("s", dst[:], shared("mu2").rearrange("p b (w t) -> p b t w", t=T))
-                give(("mu2", q, r))
+                copy(sorter, dst[:], shared("mu2").rearrange("p b (w t) -> p b t w", t=T))
+                if q == 0 or r == 1:
+                    give(("mu2", q, r if q == 0 else 0))
 
             def multiply():
                 prod = take(("prod2", j, q, r), "small", [P, 2, T, P], F32)
@@ -169,13 +180,13 @@ def tile_gaussian_nn_htanh_v_kernel(
 
             def turn():
                 prod = tiles["prod2", j, q, r]
-                mean = tiles["mean2", q, r] if q == 0 else shared("mu2").rearrange("p b (w t) -> p b t w", t=T)
+                mean = tiles["mean2", q, r] if q < SORTED else shared("mu2").rearrange("p b (w t) -> p b t w", t=T)
                 banks = [take(("w2bank", j, q, r, b), "bank", [P, T, P], F32) for b in range(2)]
                 turn_sum(banks, lambda b, t: mean[:, b, t, :], lambda b, t: prod[:, b, t, :], mean_first)
                 give(("prod2", j, q, r))
-                if j == J - 1 and q == 0:
+                if j == J - 1 and q < SORTED:
                     give(("mean2", q, r))
-                if q == 1:
+                if q >= SORTED:
                     release("mu2")
 
             def empty():
@@ -188,11 +199,13 @@ def tile_gaussian_nn_htanh_v_kernel(
                     copy(readers[b], dst[:, :, blocks, :, :], src)
                     give(("w2bank", j, q, r, b))
 
-            steps = [(-AHEAD, MAKE, multiply), (0, PE, turn), (1, READ, empty)]
+            steps = [(-ahead, MAKE, multiply), (0, PE, turn), (1, READ, empty)]
             if split or r == 0:
                 steps.append((-LEAD - AHEAD, DMA, fetch))
-            if split:
+            if j == 0 and q < SORTED:
                 steps.append((-AHEAD, MAKE, sort_mean))
+            if split and r == 0:
+                steps.append((-1, PE, warm_up))
             return steps + ([quant_step(behind, ("w2", j, q), E4M3, ("w2in", j, q))] if r == 1 else [])
 
         def grad_job(j, g, behind=BEHIND, readers="ss"):
@@ -215,7 +228,7 @@ def tile_gaussian_nn_htanh_v_kernel(
                     copy(readers[a], out, tiles["gbank", j, g, a][:].rearrange("p s u m -> p s m u"))
                     give(("gbank", j, g, a))
 
-            return [(-LEAD, DMA, fetch), (0, PE, turn), (1, READ, empty), quant_step(behind, ("g", j, g), E5M2, ("gin", j, g))]
+            return [(-LEAD - 1, DMA, fetch), (0, PE, turn), (1, READ, empty), quant_step(behind, ("g", j, g), E5M2, ("gin", j, g))]
 
         def x_job(g, half, engines, behind=3):
             def fetch():
@@ -223,16 +236,13 @@ def tile_gaussian_nn_htanh_v_kernel(
 
             def interleave(n):
                 if n == 0:
-                    take(("xin", g, half), "small", [P, K, T], BF16, newest=engines == "gg")
+                    take(("xin", g, half), "small", [P, K, T], BF16, newest=engines[0] == "g")
                 src = tiles["x", g, half][:, :, cols(n, 256)].rearrange("p t w -> p w t")
                 copy(engines[n], tiles["xin", g, half][:, cols(n, 256), :], src)
                 if n == 1:
                     give(("x", g, half))
 
-            if engines == "gg":
-                steps = [(0, POOL, partial(interleave, n)) for n in range(2)]
-            else:
-                steps = [(n, MAKE, partial(interleave, n)) for n in range(2)]
+            steps = [(0, POOL, partial(interleave, n)) if engines[n] == "g" else (n, MAKE, partial(interleave, n)) for n in range(2)]
             return steps + [(-LEAD, DMA, fetch), quant_step(behind, ("xq", g, half), E4M3, ("xin", g, half))]
 
         def w1_job(i, j, mean_first, pool_ahead=None, readers="ss", sorter="v", behind=BEHIND, ahead=AHEAD):
@@ -290,7 +300,7 @@ def tile_gaussian_nn_htanh_v_kernel(
                 steps += [quant_step(behind + q, ("w1", j, q, xh), E4M3, ("w1in", j, q, xh)) for q in range(2)]
             return steps
 
-        def dh_job(j, q, g, half, abs_ahead, markers):
+        def dh_job(j, q, g, half, abs_ahead, markers, soon):
             key = (j, q, g)
             pieces = [(0, 2), (2, 2)] if markers[2] == markers[3] else [(0, 2), (2, 1), (3, 1)]
 
@@ -338,7 +348,7 @@ def tile_gaussian_nn_htanh_v_kernel(
                     at = (-abs_ahead, POOL) if markers[u] == "g" else (-abs_ahead + 1 + u // 2, MAKE)
                     steps.append(at + (partial(mark, u, n),))
                 return steps
-            return steps + [(1, READ, mask), quant_step(2, ("dzn",) + key, E5M2, ("dz",) + key, False)]
+            return steps + [(1, READ, mask), quant_step(soon, ("dzn",) + key, E5M2, ("dz",) + key, False)]
 
         def dzt_job(j, q, g, behind):
             key = (j, q, g)
@@ -360,7 +370,7 @@ def tile_gaussian_nn_htanh_v_kernel(
 
             return [(0, PE, turn), (1, READ, empty), quant_step(behind, ("dzh",) + key, E5M2, ("dzin",) + key)]
 
-        def dx_job(g, xh, t, width=2, passes=range(4), reader="s"):
+        def dx_job(g, xh, t, width=2, passes=range(4), reader="s", queue=nc.sync):
             pair = (g, xh, t // width)
 
             def multiply():
@@ -383,7 +393,7 @@ def tile_gaussian_nn_htanh_v_kernel(
 
             def store():
                 dst = out_0.rearrange("(g p t) w -> g p t w", g=2, t=T)[g][:, cols(t // width, width), cols(xh, K)]
-                nc.sync.dma_start(out=dst, in_=tiles[("out0",) + pair][:])
+                queue.dma_start(out=dst, in_=tiles[("out0",) + pair][:])
                 give(("out0",) + pair)
 
             if 3 not in passes:
@@ -429,8 +439,28 @@ def tile_gaussian_nn_htanh_v_kernel(
             steps = [(0, PE, multiply), (1, READ, weigh), (1, MAKE, lambda: [add(i) for i in done])]
             return steps + [(store_behind, DMA, lambda: [store(i) for i in done if i % 2 == 1])]
 
-        def dx_jobs(g, xh, width=2, passes=range(4)):
-            return [dx_job(g, xh, t, width, passes) for t in range(T)]
+        def dx_last(g, xh, t, part, reader):
+            key = ("dx", g, xh, t, part)
+
+            def multiply():
+                bank = take(key, "bank", [P, K // 2], F32)
+                for k in range(4):
+                    q, j = divmod(k, 2)
+                    mx(bank[:], ("dzh", j, q, g), cols(t), E5M2, ("w1", j, q, xh), cols(part, K // 2), E4M3, k == 0, k == 3)
+
+            def empty():
+                copy(reader, take(("out0",) + key, "small", [P, K // 2], F32)[:], tiles[key][:])
+                give(key)
+
+            def store():
+                dst = out_0.rearrange("(g p t) w -> g p t w", g=2, t=T)[g][:, t, cols(2 * xh + part, K // 2)]
+                (nc.scalar if reader == "s" else nc.sync).dma_start(out=dst, in_=tiles[("out0",) + key][:])
+                give(("out0",) + key)
+
+            return [(0, PE, multiply), (1, READ, empty), (1, DMA, store)]
+
+        def dx_jobs(g, xh, width=2, passes=range(4), queue=nc.sync):
+            return [dx_job(g, xh, t, width, passes, "s", queue) for t in range(T)]
 
         def dw_jobs(q, j, engine):
             return [dw_job(q, [(i, j), (i + 1, j)], engine) for i in range(0, 8, 2)]
@@ -438,10 +468,10 @@ def tile_gaussian_nn_htanh_v_kernel(
         jobs = []
         starts = []
 
-        def unit(key, markers, early, late, behind=BEHIND, beside=()):
-            ahead = len(jobs) - starts[-1] - 1 if starts else 2
+        def unit(key, markers, early, late, behind=BEHIND, beside=(), soon=2):
+            ahead = len(jobs) - starts[-1] - 1 if starts else 3
             starts.append(len(jobs))
-            jobs.extend([dh_job(*key, 0, ahead, markers), dh_job(*key, 1, ahead, markers) + list(beside)] + early + [dzt_job(*key, behind)] + late)
+            jobs.extend([dh_job(*key, 0, ahead, markers, soon), dh_job(*key, 1, ahead, markers, soon) + list(beside)] + early + [dzt_job(*key, behind)] + late)
 
         def weave(first, second):
             jobs = []
@@ -457,20 +487,20 @@ def tile_gaussian_nn_htanh_v_kernel(
 
         jobs.extend([w2_job(0, 0, 0, False), w2_job(0, 0, 1, True, 2), grad_job(0, 0, 1, "vv"), w2_job(1, 0, 0, False)])
         unit(order[0], "ssss", [w2_job(1, 0, 1, True), grad_job(1, 0)], [w2_job(0, 1, 0, False), w2_job(0, 1, 1, True), w2_job(1, 1, 0, False)], 5)
-        unit(order[1], "gggg", [w2_job(1, 1, 1, True), w1(0, False), w1(1, True, 3)], [w1(2, False)], 3)
+        unit(order[1], "gggg", [w2_job(1, 1, 1, True), w1(0, False), w1(1, True, 3)], [w1(2, True)], 3)
         unit(order[2], "ssss", [w1(3, True), w1(4, False), w1(5, True, 3, "vs")], [w1(6, False), w1(7, False)], 4)
         unit(order[3], "ssss", [w1(8, True), grad_job(0, 1, 4), w1(9, True)], [w1(10, False) + x_job(0, 1, "vv"), w1(11, True), grad_job(1, 1, 5)], 5, x_job(0, 0, "gg", 5))
         dx = dx_jobs(0, 0)
-        unit(order[4], "ssss", [dx[0], dx[1], w1(12, True)], [w1(13, False), dx[2] + x_job(1, 1, "vv", 3), dx[3]], 5, x_job(1, 0, "gg", 5))
+        unit(order[4], "ssss", [dx[0], dx[1], w1(12, True)], [w1(13, True), dx[2] + x_job(1, 1, "vv", 3), dx[3]], 5, x_job(1, 0, "gg", 5))
         dw = dw_jobs(0, 0, "g")
-        unit(order[5], "ssss", [dw[0], dw[1], w1(14, True, 3)], [w1(15, False, 3), dw[2], dw[3]], 5)
+        unit(order[5], "ssss", [dw[0], dw[1], w1(14, True, 3)], [w1(15, True, 3), dw[2], dw[3]], 5, soon=3)
         dx = dx_jobs(0, 1)
         dw = dw_jobs(0, 1, "g")
-        unit(order[6], "ssss", dw[:2] + dx[:1], weave(dw[2:], dx[1:]), 3)
+        unit(order[6], "ssss", dw[:2] + dx[:1], weave(dw[2:], dx[1:]), 3, soon=2)
         both = [(i, 0) for i in range(4)] + [(i, 1) for i in range(4)] + [(i, j) for i in range(4, 8) for j in range(J)]
         dw = [dw_job(1, both[n : n + 2], "vgvggggg", 3) for n in range(0, 16, 2)]
-        unit(order[7], "ssss", dw[:2], dw[2:5], 2)
-        jobs.extend(weave(dx_jobs(1, 0) + dx_jobs(1, 1, 1), dw[5:]))
+        unit(order[7], "ssss", dw[:2], dw[2:6], 2, soon=1)
+        jobs.extend(weave(dx_jobs(1, 0, 1) + dx_jobs(1, 1, 1)[:3] + [dx_last(1, 1, 3, 0, "s"), dx_last(1, 1, 3, 1, "v")], dw[6:]))
 
         steps = []
         for tick in range(len(jobs)):

@@ -32,6 +32,8 @@ AHEAD = 2
 BEHIND = 3
 SORTED = 1
 WARM = 0
+ADD_PIECES = 1
+POOL_PART = 3
 
 
 def tile_gaussian_nn_htanh_v_kernel(
@@ -262,16 +264,16 @@ def tile_gaussian_nn_htanh_v_kernel(
                 copy(sorter, dst[:], tiles["mu1", a][:].rearrange("p r (b t i) -> p r t b i", t=T, i=8))
                 give(("mu1", a))
 
-            def multiply():
-                prod = take(("prod1", i, j), "small", [P, T, 32, 8], F32, newest=pool_ahead is not None)
-                eng = nc.vector if pool_ahead is None else nc.gpsimd
+            def multiply(eng, part):
+                if part.start == 0:
+                    take(("prod1", i, j), "small", [P, T, 32, 8], F32, newest=pool_ahead is not None)
                 eng.tensor_tensor(
-                    out=prod[:],
-                    in0=tiles["e1", i][:, j, :].rearrange(order, t=T, i=8),
-                    in1=tiles["sig1", a][:, r, :].rearrange(order, t=T, i=8),
+                    out=tiles["prod1", i, j][:, part],
+                    in0=tiles["e1", i][:, j, :].rearrange(order, t=T, i=8)[:, part],
+                    in1=tiles["sig1", a][:, r, :].rearrange(order, t=T, i=8)[:, part],
                     op=ALU.mult,
                 )
-                if r == 1 and j == J - 1:
+                if r == 1 and j == J - 1 and part.stop == T:
                     give(("sig1", a))
 
             def turn():
@@ -291,7 +293,13 @@ def tile_gaussian_nn_htanh_v_kernel(
                     copy(readers[q], tiles["w1in", j, q, xh][:, cols(c), :], src)
                     give(("w1bank", i, j, q))
 
-            steps = [(-ahead, MAKE, multiply) if pool_ahead is None else (-pool_ahead, POOL, multiply), (0, PE, turn), (1, READ, empty)]
+            steps = [(0, PE, turn), (1, READ, empty)]
+            if pool_ahead is None:
+                steps.append((-ahead, MAKE, partial(multiply, nc.vector, slice(0, T))))
+            else:
+                steps.append((-pool_ahead, POOL, partial(multiply, nc.gpsimd, slice(0, POOL_PART))))
+                if POOL_PART < T:
+                    steps.append((-pool_ahead + 1, MAKE, partial(multiply, nc.vector, slice(POOL_PART, T))))
             if j == 0:
                 steps.append((-LEAD - AHEAD, DMA, fetch))
                 if r == 0:
@@ -426,7 +434,10 @@ def tile_gaussian_nn_htanh_v_kernel(
             def add(i):
                 first, second = tiles["part", q, i // 2, 0][:, i % 2, :], tiles["part", q, i // 2, 1][:, i % 2, :]
                 eng = nc.gpsimd if engine[i % len(engine)] == "g" else nc.vector
-                eng.tensor_tensor(out=first, in0=first, in1=second, op=ALU.add)
+                pieces = ADD_PIECES if eng is nc.gpsimd else 1
+                for n in range(pieces):
+                    part = cols(n, K // pieces)
+                    eng.tensor_tensor(out=first[:, part], in0=first[:, part], in1=second[:, part], op=ALU.add)
                 if i % 2 == 1:
                     give(("part", q, i // 2, 1))
 
@@ -468,8 +479,8 @@ def tile_gaussian_nn_htanh_v_kernel(
         jobs = []
         starts = []
 
-        def unit(key, markers, early, late, behind=BEHIND, beside=(), soon=2):
-            ahead = len(jobs) - starts[-1] - 1 if starts else 3
+        def unit(key, markers, early, late, behind=BEHIND, beside=(), soon=2, ahead=None):
+            ahead = ahead or (len(jobs) - starts[-1] - 1 if starts else 3)
             starts.append(len(jobs))
             jobs.extend([dh_job(*key, 0, ahead, markers, soon), dh_job(*key, 1, ahead, markers, soon) + list(beside)] + early + [dzt_job(*key, behind)] + late)
 
@@ -487,16 +498,16 @@ def tile_gaussian_nn_htanh_v_kernel(
 
         jobs.extend([w2_job(0, 0, 0, False), w2_job(0, 0, 1, True, 2), grad_job(0, 0, 1, "vv"), w2_job(1, 0, 0, False)])
         unit(order[0], "ssss", [w2_job(1, 0, 1, True), grad_job(1, 0)], [w2_job(0, 1, 0, False), w2_job(0, 1, 1, True), w2_job(1, 1, 0, False)], 5)
-        unit(order[1], "gggg", [w2_job(1, 1, 1, True), w1(0, False), w1(1, True, 3)], [w1(2, True)], 3)
+        unit(order[1], "ssss", [w2_job(1, 1, 1, True), w1(0, False), w1(1, True, 3)], [w1(2, False)], 3, ahead=4)
         unit(order[2], "ssss", [w1(3, True), w1(4, False), w1(5, True, 3, "vs")], [w1(6, False), w1(7, False)], 4)
-        unit(order[3], "ssss", [w1(8, True), grad_job(0, 1, 4), w1(9, True)], [w1(10, False) + x_job(0, 1, "vv"), w1(11, True), grad_job(1, 1, 5)], 5, x_job(0, 0, "gg", 5))
+        unit(order[3], "ssss", [w1(8, True), grad_job(0, 1, 4), w1(9, True)], [w1(10, False) + x_job(0, 1, "vv"), w1(11, True), grad_job(1, 1, 5)], 5, x_job(0, 0, "gv", 5))
         dx = dx_jobs(0, 0)
-        unit(order[4], "ssss", [dx[0], dx[1], w1(12, True)], [w1(13, True), dx[2] + x_job(1, 1, "vv", 3), dx[3]], 5, x_job(1, 0, "gg", 5))
+        unit(order[4], "ssss", [dx[0], dx[1], w1(12, True)], [w1(13, False), dx[2] + x_job(1, 1, "vv", 3), dx[3]], 5, x_job(1, 0, "gv", 5))
         dw = dw_jobs(0, 0, "g")
-        unit(order[5], "ssss", [dw[0], dw[1], w1(14, True, 3)], [w1(15, True, 3), dw[2], dw[3]], 5, soon=3)
+        unit(order[5], "ssss", [dw[0], dw[1], w1(14, True, 3)], [w1(15, False, 3), dw[2], dw[3]], 5, soon=3)
         dx = dx_jobs(0, 1)
         dw = dw_jobs(0, 1, "g")
-        unit(order[6], "ssss", dw[:2] + dx[:1], weave(dw[2:], dx[1:]), 3, soon=2)
+        unit(order[6], "ssss", dw[:2] + dx[:1], weave(dw[2:], dx[1:]), 3, soon=1)
         both = [(i, 0) for i in range(4)] + [(i, 1) for i in range(4)] + [(i, j) for i in range(4, 8) for j in range(J)]
         dw = [dw_job(1, both[n : n + 2], "vgvggggg", 3) for n in range(0, 16, 2)]
         unit(order[7], "ssss", dw[:2], dw[2:6], 2, soon=1)

@@ -32,6 +32,8 @@ AHEAD = 2
 BEHIND = 3
 SORTED = 1
 WARM = 0
+X_WHOLE = False
+MU_LATE = 0
 ADD_PIECES = 1
 POOL_PART = 3
 
@@ -123,38 +125,34 @@ def tile_gaussian_nn_htanh_v_kernel(
         def cols(n, width=P):
             return slice(width * n, width * n + width)
 
-        def turn_sum(banks, mean_of, prod_of, mean_first):
-            for second in (False, True):
-                for b in range(2):
-                    for t in range(T):
-                        flags = dict(start=(t == 0 and not second), stop=(t == T - 1 and second))
-                        if mean_first != second:
-                            nc.tensor.matmul(banks[b][:, t, :], lhsT=mean_of(b, t), rhs=ident_b[:], **flags)
-                        else:
-                            nc.tensor.matmul(banks[b][:, t, :], lhsT=prod_of(b, t), rhs=ident_f[:], is_transpose=True, **flags)
+        def turn_sum(banks, mean_of, prod_of, mean_first, second):
+            for b in range(2):
+                for t in range(T):
+                    flags = dict(start=(t == 0 and not second), stop=(t == T - 1 and second))
+                    if mean_first != second:
+                        nc.tensor.matmul(banks[b][:, t, :], lhsT=mean_of(b, t), rhs=ident_b[:], **flags)
+                    else:
+                        nc.tensor.matmul(banks[b][:, t, :], lhsT=prod_of(b, t), rhs=ident_f[:], is_transpose=True, **flags)
+
+        def turn_steps(turn, empty, shift):
+            return [(min(shift, 0), PE, partial(turn, False)), (max(shift, 0), PE, partial(turn, True)), (max(shift, 0) + 1, READ, empty)]
 
         PE, READ, MAKE, QUANT, POOL, DMA = range(6)
 
-        def w2_job(j, q, r, mean_first, behind=BEHIND, readers="ss", sorter="s", ahead=AHEAD):
-            split = j == 0 and q == 0
+        def w2_job(j, q, r, mean_first, behind=BEHIND, readers="ss", sorter="s", ahead=AHEAD, shift=0):
+            split = q == 0
             part = r if split else 0
 
-            def rows(key):
-                return tiles[key + (part,)][:, cols(0 if split else r, 2), :]
+            def shared(*name):
+                return tiles[name + (q, part)][:, cols(0 if split else r, 2), :]
 
-            def fetch():
-                wanted = [(("sig2", q), sig_W2), (("e2", j, q), e_W2[j]), (("mu2", q), mu_W2)]
-                for key, src in wanted if j == 0 else wanted[1:2]:
-                    blocks = 2 if split else 4
-                    view = src.rearrange("(a b m) y -> a m b y", b=blocks, m=P)[2 * q + r if split else q]
-                    load(key + (part,), "small", [P, blocks, Y], BF16, view)
+            def fetch(src, *name):
+                view = src.rearrange("(a b m) y -> a m b y", b=2 if split else 4, m=P)[r if split else q]
+                load(name + (q, part), "small", [P, 2 if split else 4, Y], BF16, view)
 
-            def shared(name):
-                return tiles[name, q, r][:] if q == 0 else tiles[name, q, 0][:, cols(r, 2), :]
-
-            def release(name):
-                if j == J - 1 and (q == 0 or r == 1):
-                    give((name, q, r if q == 0 else 0))
+            def release(*name):
+                if split or r == 1:
+                    give(name + (q, part))
 
             def warm_up():
                 for n in range(WARM):
@@ -167,28 +165,29 @@ def tile_gaussian_nn_htanh_v_kernel(
             def sort_mean():
                 dst = take(("mean2", q, r), "small", [P, 2, T, P], BF16)
                 copy(sorter, dst[:], shared("mu2").rearrange("p b (w t) -> p b t w", t=T))
-                if q == 0 or r == 1:
-                    give(("mu2", q, r if q == 0 else 0))
+                release("mu2")
 
             def multiply():
                 prod = take(("prod2", j, q, r), "small", [P, 2, T, P], F32)
                 order = "p b (w t) -> p b t w"
                 nc.vector.tensor_tensor(
-                    out=prod[:], in0=rows(("e2", j, q)).rearrange(order, t=T), in1=shared("sig2").rearrange(order, t=T), op=ALU.mult
+                    out=prod[:], in0=shared("e2", j).rearrange(order, t=T), in1=shared("sig2").rearrange(order, t=T), op=ALU.mult
                 )
-                if split or r == 1:
-                    give(("e2", j, q, part))
-                release("sig2")
+                release("e2", j)
+                if j == J - 1:
+                    release("sig2")
 
-            def turn():
-                prod = tiles["prod2", j, q, r]
+            def turn(second):
+                prod = tiles.get(("prod2", j, q, r))
                 mean = tiles["mean2", q, r] if q < SORTED else shared("mu2").rearrange("p b (w t) -> p b t w", t=T)
-                banks = [take(("w2bank", j, q, r, b), "bank", [P, T, P], F32) for b in range(2)]
-                turn_sum(banks, lambda b, t: mean[:, b, t, :], lambda b, t: prod[:, b, t, :], mean_first)
+                banks = [tiles["w2bank", j, q, r, b] if second else take(("w2bank", j, q, r, b), "bank", [P, T, P], F32) for b in range(2)]
+                turn_sum(banks, lambda b, t: mean[:, b, t, :], lambda b, t: prod[:, b, t, :], mean_first, second)
+                if not second:
+                    return
                 give(("prod2", j, q, r))
                 if j == J - 1 and q < SORTED:
                     give(("mean2", q, r))
-                if q >= SORTED:
+                if q >= SORTED and j == J - 1:
                     release("mu2")
 
             def empty():
@@ -201,12 +200,15 @@ def tile_gaussian_nn_htanh_v_kernel(
                     copy(readers[b], dst[:, :, blocks, :, :], src)
                     give(("w2bank", j, q, r, b))
 
-            steps = [(-ahead, MAKE, multiply), (0, PE, turn), (1, READ, empty)]
+            steps = [(-ahead, MAKE, multiply)] + turn_steps(turn, empty, shift)
             if split or r == 0:
-                steps.append((-LEAD - AHEAD, DMA, fetch))
+                if j == 0:
+                    steps.append((-LEAD - AHEAD, DMA, partial(fetch, sig_W2, "sig2")))
+                    steps.append((-LEAD - AHEAD + MU_LATE, DMA + MU_LATE, partial(fetch, mu_W2, "mu2")))
+                steps.append((-LEAD - AHEAD, DMA, partial(fetch, e_W2[j], "e2", j)))
             if j == 0 and q < SORTED:
-                steps.append((-AHEAD, MAKE, sort_mean))
-            if split and r == 0:
+                steps.append((-ahead - (1 + r if q else 0), MAKE, sort_mean))
+            if split and r == 0 and j == 0:
                 steps.append((-1, PE, warm_up))
             return steps + ([quant_step(behind, ("w2", j, q), E4M3, ("w2in", j, q))] if r == 1 else [])
 
@@ -234,20 +236,25 @@ def tile_gaussian_nn_htanh_v_kernel(
 
         def x_job(g, half, engines, behind=3):
             def fetch():
+                if X_WHOLE:
+                    load(("x", g), "large", [P, T, X], BF16, x.rearrange("(g p t) w -> g p t w", g=2, t=T)[g])
+                    return
                 load(("x", g, half), "small", [P, T, K], BF16, x.rearrange("(g p t) w -> g p t w", g=2, t=T)[g][:, :, cols(half, K)])
 
             def interleave(n):
                 if n == 0:
                     take(("xin", g, half), "small", [P, K, T], BF16, newest=engines[0] == "g")
-                src = tiles["x", g, half][:, :, cols(n, 256)].rearrange("p t w -> p w t")
+                src = (tiles["x", g][:, :, cols(2 * half + n, 256)] if X_WHOLE else tiles["x", g, half][:, :, cols(n, 256)]).rearrange("p t w -> p w t")
                 copy(engines[n], tiles["xin", g, half][:, cols(n, 256), :], src)
-                if n == 1:
+                if n == 1 and not X_WHOLE:
                     give(("x", g, half))
+                if n == 1 and X_WHOLE and half == 1:
+                    give(("x", g))
 
             steps = [(0, POOL, partial(interleave, n)) if engines[n] == "g" else (n, MAKE, partial(interleave, n)) for n in range(2)]
-            return steps + [(-LEAD, DMA, fetch), quant_step(behind, ("xq", g, half), E4M3, ("xin", g, half))]
+            return steps + ([] if X_WHOLE and half else [(-LEAD, DMA, fetch)]) + [quant_step(behind, ("xq", g, half), E4M3, ("xin", g, half))]
 
-        def w1_job(i, j, mean_first, pool_ahead=None, readers="ss", sorter="v", behind=BEHIND, ahead=AHEAD):
+        def w1_job(i, j, mean_first, pool_ahead=None, readers="ss", sorter="v", behind=BEHIND, ahead=AHEAD, shift=0):
             a, r = divmod(i, 2)
             xh, c = divmod(i, 4)
             order = "p (b t i) -> p t b i"
@@ -276,14 +283,40 @@ def tile_gaussian_nn_htanh_v_kernel(
                 if r == 1 and j == J - 1 and part.stop == T:
                     give(("sig1", a))
 
-            def turn():
+            def turn(second):
                 prod = tiles["prod1", i, j][:].rearrange("p t (q b) i -> p t q (b i)", q=2)
                 mean = tiles["mean1", a][:, r].rearrange("p t (q b) i -> p t q (b i)", q=2)
-                banks = [take(("w1bank", i, j, q), "bank", [P, T, P], F32) for q in range(2)]
-                turn_sum(banks, lambda q, t: mean[:, t, q, :], lambda q, t: prod[:, t, q, :], mean_first)
+                banks = [tiles["w1bank", i, j, q] if second else take(("w1bank", i, j, q), "bank", [P, T, P], F32) for q in range(2)]
+                turn_sum(banks, lambda q, t: mean[:, t, q, :], lambda q, t: prod[:, t, q, :], mean_first, second)
+                if not second:
+                    return
                 give(("prod1", i, j))
                 if r == 1 and j == J - 1:
                     give(("mean1", a))
+
+            def add_mean(eng):
+                total = take(("sum1", i, j), "small", [P, 2, 256, 2], BF16)
+                pairs = "p (s e) b i -> p s (b i) e"
+                eng.tensor_tensor(out=total[:], in0=tiles["prod1", i, j][:].rearrange(pairs, e=2), in1=tiles["mean1", a][:, r].rearrange(pairs, e=2), op=ALU.add)
+                give(("prod1", i, j))
+                if r == 1 and j == J - 1:
+                    give(("mean1", a))
+
+            def turn_words():
+                words = tiles["sum1", i, j][:].rearrange("p s n e -> p (s n e)").bitcast(F32).rearrange("p (s q n) -> p s q n", s=2, q=2)
+                bank = take(("w1bank", i, j), "bank", [P, 2, 2, P], F32)
+                for q in range(2):
+                    for s in range(2):
+                        nc.tensor.transpose(bank[:, q, s, :], words[:, s, q, :], ident_f[:])
+                give(("sum1", i, j))
+
+            def empty_words():
+                for q in range(2):
+                    if c == 0:
+                        take(("w1in", j, q, xh), "small", [P, K, T], BF16)
+                    dst = tiles["w1in", j, q, xh][:, cols(c), :].rearrange("p m t -> p (m t)").bitcast(F32).rearrange("p (m s) -> p m s", s=2)
+                    copy(readers[q], dst, tiles["w1bank", i, j][:, q].rearrange("p s m -> p m s"))
+                give(("w1bank", i, j))
 
             def empty():
                 for q in range(2):
@@ -293,7 +326,9 @@ def tile_gaussian_nn_htanh_v_kernel(
                     copy(readers[q], tiles["w1in", j, q, xh][:, cols(c), :], src)
                     give(("w1bank", i, j, q))
 
-            steps = [(0, PE, turn), (1, READ, empty)]
+            steps = turn_steps(turn, empty, shift)
+            if mean_first is None:
+                steps = [(-1, MAKE, partial(add_mean, nc.vector)), (0, PE, turn_words), (1, READ, empty_words)]
             if pool_ahead is None:
                 steps.append((-ahead, MAKE, partial(multiply, nc.vector, slice(0, T))))
             else:
@@ -311,9 +346,20 @@ def tile_gaussian_nn_htanh_v_kernel(
         def dh_job(j, q, g, half, abs_ahead, markers, soon):
             key = (j, q, g)
             pieces = [(0, 2), (2, 2)] if markers[2] == markers[3] else [(0, 2), (2, 1), (3, 1)]
+            if markers == "llll":
+                pieces = [(0, 4)]
 
             def fetch():
                 load(("z",) + key, "large", [P, T, K], F32, z1[j].rearrange("(g p t) h -> g p t h", g=2, t=T)[g][:, :, cols(q, K)])
+
+            def mark_lines(n):
+                if n == 0:
+                    take(("mark",) + key + (0,), "small", [P, 16, 32, T], BF16)
+                dst = tiles[("mark",) + key + (0,)][:].rearrange("p b (c i) t -> p (b c) t i", i=4)[:, cols(n, 64)]
+                src = tiles[("z",) + key][:].rearrange("p t (c i) -> p c t i", i=4)[:, cols(n, 64)]
+                nc.scalar.activation(out=dst, in_=src, func=ACT.Abs, scale=EDGE)
+                if n == 1:
+                    give(("z",) + key)
 
             def mark(u, n):
                 src = tiles[("z",) + key][:].rearrange("p t (b h) -> p b h t", h=32)[:, :, 8 * u : 8 * (u + n), :]
@@ -343,7 +389,7 @@ def tile_gaussian_nn_htanh_v_kernel(
                     bank = tiles[("dh",) + key + (u,)][:].rearrange("p t (b i) -> p b i t", i=8)
                     first, n = [piece for piece in pieces if piece[0] <= u][-1]
                     marks = tiles[("mark",) + key + (first,)][:, :, cols(u - first, 8), :]
-                    level, test = (EDGE, ALU.is_lt) if markers[u] == "s" else (CENTRE, ALU.is_equal)
+                    level, test = (EDGE, ALU.is_lt) if markers[u] != "g" else (CENTRE, ALU.is_equal)
                     nc.vector.scalar_tensor_tensor(out=dz[:, u], in0=marks, scalar=level, in1=bank, op0=test, op1=ALU.mult)
                     give(("dh",) + key + (u,))
                     if u == first + n - 1:
@@ -352,22 +398,34 @@ def tile_gaussian_nn_htanh_v_kernel(
             steps = [(0, PE, multiply)]
             if half == 0:
                 steps.append((-LEAD - abs_ahead, DMA, fetch))
+                if markers == "llll":
+                    return steps + [(-abs_ahead + 1 + n, MAKE, partial(mark_lines, n)) for n in range(2)]
                 for u, n in pieces:
                     at = (-abs_ahead, POOL) if markers[u] == "g" else (-abs_ahead + 1 + u // 2, MAKE)
                     steps.append(at + (partial(mark, u, n),))
                 return steps
             return steps + [(1, READ, mask), quant_step(soon, ("dzn",) + key, E5M2, ("dz",) + key, False)]
 
-        def dzt_job(j, q, g, behind):
+        def dzt_job(j, q, g, behind, presort):
             key = (j, q, g)
 
+            def pairs():
+                return tiles[("dz",) + key][:].rearrange("p c t -> p (c t)").bitcast(F32).rearrange("p (u m s) -> p s u m", u=T, s=2)
+
+            def sort(s):
+                if s == 0:
+                    take(("dzw",) + key, "small", [P, 2, T, P], F32)
+                copy(presort, tiles[("dzw",) + key][:, s], pairs()[:, s])
+
             def turn():
-                words = tiles[("dz",) + key][:].rearrange("p c t -> p (c t)").bitcast(F32).rearrange("p (u m s) -> p u m s", u=T, s=2)
+                words = tiles[("dzw",) + key][:] if presort else pairs()
                 for s in range(2):
                     bank = take(("dzbank",) + key + (s,), "bank", [P, T, P], F32)
                     for u in range(T):
-                        nc.tensor.transpose(bank[:, u, :], words[:, u, :, s], ident_f[:])
+                        nc.tensor.transpose(bank[:, u, :], words[:, s, u, :], ident_f[:])
                 give(("dz",) + key)
+                if presort:
+                    give(("dzw",) + key)
 
             def empty():
                 dst = take(("dzin",) + key, "small", [P, K, T], BF16)
@@ -376,7 +434,8 @@ def tile_gaussian_nn_htanh_v_kernel(
                     nc.scalar.copy(out=dst[:, cols(s, 256), :].rearrange("p (e m) u -> p e m u", e=2), in_=src)
                     give(("dzbank",) + key + (s,))
 
-            return [(0, PE, turn), (1, READ, empty), quant_step(behind, ("dzh",) + key, E5M2, ("dzin",) + key)]
+            steps = [(-1, READ, partial(sort, s)) for s in range(2)] if presort else []
+            return steps + [(0, PE, turn), (1, READ, empty), quant_step(behind, ("dzh",) + key, E5M2, ("dzin",) + key)]
 
         def dx_job(g, xh, t, width=2, passes=range(4), reader="s", queue=nc.sync):
             pair = (g, xh, t // width)
@@ -479,10 +538,10 @@ def tile_gaussian_nn_htanh_v_kernel(
         jobs = []
         starts = []
 
-        def unit(key, markers, early, late, behind=BEHIND, beside=(), soon=2, ahead=None):
+        def unit(key, markers, early, late, behind=BEHIND, beside=(), soon=2, ahead=None, presort=None):
             ahead = ahead or (len(jobs) - starts[-1] - 1 if starts else 3)
             starts.append(len(jobs))
-            jobs.extend([dh_job(*key, 0, ahead, markers, soon), dh_job(*key, 1, ahead, markers, soon) + list(beside)] + early + [dzt_job(*key, behind)] + late)
+            jobs.extend([dh_job(*key, 0, ahead, markers, soon), dh_job(*key, 1, ahead, markers, soon) + list(beside)] + early + [dzt_job(*key, behind, presort)] + late)
 
         def weave(first, second):
             jobs = []
@@ -493,24 +552,24 @@ def tile_gaussian_nn_htanh_v_kernel(
         order = [(j, q, g) for g in range(2) for q in range(2) for j in range(J)]
         first = dx_jobs(0, 0) + dx_jobs(0, 1)
         first = dx_jobs(0, 0) + dx_jobs(0, 1)
-        def w1(n, mean_first, pool_ahead=None, readers="ss", behind=BEHIND, ahead=3, sorter="v"):
-            return w1_job(n // 2, n % 2, mean_first, pool_ahead, readers, sorter, behind, ahead)
+        def w1(n, mean_first, shift=0, pool_ahead=None, readers="ss", behind=BEHIND, ahead=3, sorter="v"):
+            return w1_job(n // 2, n % 2, mean_first, pool_ahead, readers, sorter, behind, ahead, shift)
 
         jobs.extend([w2_job(0, 0, 0, False), w2_job(0, 0, 1, True, 2), grad_job(0, 0, 1, "vv"), w2_job(1, 0, 0, False)])
         unit(order[0], "ssss", [w2_job(1, 0, 1, True), grad_job(1, 0)], [w2_job(0, 1, 0, False), w2_job(0, 1, 1, True), w2_job(1, 1, 0, False)], 5)
-        unit(order[1], "ssss", [w2_job(1, 1, 1, True), w1(0, False), w1(1, True, 3)], [w1(2, False)], 3, ahead=4)
-        unit(order[2], "ssss", [w1(3, True), w1(4, False), w1(5, True, 3, "vs")], [w1(6, False), w1(7, False)], 4)
-        unit(order[3], "ssss", [w1(8, True), grad_job(0, 1, 4), w1(9, True)], [w1(10, False) + x_job(0, 1, "vv"), w1(11, True), grad_job(1, 1, 5)], 5, x_job(0, 0, "gv", 5))
+        unit(order[1], "llll", [w2_job(1, 1, 1, True), w1(0, False), w1(1, True, 0, 3)], [w1(2, False)], 3, ahead=4)
+        unit(order[2], "llll", [w1(3, True), w1(4, False), w1(5, True, 0, 3, "vs")], [w1(6, False), w1(7, False)], 4)
+        unit(order[3], "llll", [w1(8, True), grad_job(0, 1, 4), w1(9, True)], [w1(10, False) + x_job(0, 1, "vv"), w1(11, True), grad_job(1, 1, 5)], 5, x_job(0, 0, "gv", 5))
         dx = dx_jobs(0, 0)
-        unit(order[4], "ssss", [dx[0], dx[1], w1(12, True)], [w1(13, False), dx[2] + x_job(1, 1, "vv", 3), dx[3]], 5, x_job(1, 0, "gv", 5))
+        unit(order[4], "llll", [dx[0], dx[1], w1(12, True)], [w1(13, False), dx[2] + x_job(1, 1, "vv", 3), dx[3]], 5, x_job(1, 0, "gv", 5))
         dw = dw_jobs(0, 0, "g")
-        unit(order[5], "ssss", [dw[0], dw[1], w1(14, True, 3)], [w1(15, False, 3), dw[2], dw[3]], 5, soon=3)
+        unit(order[5], "llll", [dw[0], dw[1], w1(14, True, 0, 3)], [w1(15, False, 0, 3), dw[2], dw[3]], 5, soon=3)
         dx = dx_jobs(0, 1)
         dw = dw_jobs(0, 1, "g")
-        unit(order[6], "ssss", dw[:2] + dx[:1], weave(dw[2:], dx[1:]), 3, soon=1)
+        unit(order[6], "llll", dw[:2] + dx[:1], weave(dw[2:], dx[1:]), 3, soon=1)
         both = [(i, 0) for i in range(4)] + [(i, 1) for i in range(4)] + [(i, j) for i in range(4, 8) for j in range(J)]
         dw = [dw_job(1, both[n : n + 2], "vgvggggg", 3) for n in range(0, 16, 2)]
-        unit(order[7], "ssss", dw[:2], dw[2:6], 2, soon=1)
+        unit(order[7], "llll", dw[:2], dw[2:6], 2, soon=1)
         jobs.extend(weave(dx_jobs(1, 0, 1) + dx_jobs(1, 1, 1)[:3] + [dx_last(1, 1, 3, 0, "s"), dx_last(1, 1, 3, 1, "v")], dw[6:]))
 
         steps = []

@@ -32,6 +32,10 @@ AHEAD = 2
 BEHIND = 3
 SORTED = 1
 WARM = 0
+P2_RUN = 2
+X_RUN = 4
+W_RUN = 1
+DZ_RUN = 0
 X_WHOLE = False
 MU_LATE = 0
 ADD_PIECES = 1
@@ -163,15 +167,19 @@ def tile_gaussian_nn_htanh_v_kernel(
                     give(("warm",))
 
             def sort_mean():
-                dst = take(("mean2", q, r), "small", [P, 2, T, P], BF16)
-                copy(sorter, dst[:], shared("mu2").rearrange("p b (w t) -> p b t w", t=T))
+                dst = take(("mean2", q, r), "small", [P, T, 2, P], BF16)
+                src = shared("mu2").rearrange("p b (w i t) -> p (b w) t i", t=T, i=4)
+                copy(sorter, dst[:].rearrange("p t b (w i) -> p (b w) t i", i=4), src)
                 release("mu2")
 
             def multiply():
-                prod = take(("prod2", j, q, r), "small", [P, 2, T, P], F32)
-                order = "p b (w t) -> p b t w"
+                prod = take(("prod2", j, q, r), "small", [P, T, 2, P], F32)
+                order = "p b (w i t) -> p (b w) t i"
                 nc.vector.tensor_tensor(
-                    out=prod[:], in0=shared("e2", j).rearrange(order, t=T), in1=shared("sig2").rearrange(order, t=T), op=ALU.mult
+                    out=prod[:].rearrange("p t b (w i) -> p (b w) t i", i=P2_RUN),
+                    in0=shared("e2", j).rearrange(order, t=T, i=P2_RUN),
+                    in1=shared("sig2").rearrange(order, t=T, i=P2_RUN),
+                    op=ALU.mult,
                 )
                 release("e2", j)
                 if j == J - 1:
@@ -179,9 +187,9 @@ def tile_gaussian_nn_htanh_v_kernel(
 
             def turn(second):
                 prod = tiles.get(("prod2", j, q, r))
-                mean = tiles["mean2", q, r] if q < SORTED else shared("mu2").rearrange("p b (w t) -> p b t w", t=T)
+                mean = tiles["mean2", q, r] if q < SORTED else shared("mu2").rearrange("p b (w t) -> p t b w", t=T)
                 banks = [tiles["w2bank", j, q, r, b] if second else take(("w2bank", j, q, r, b), "bank", [P, T, P], F32) for b in range(2)]
-                turn_sum(banks, lambda b, t: mean[:, b, t, :], lambda b, t: prod[:, b, t, :], mean_first, second)
+                turn_sum(banks, lambda b, t: mean[:, t, b, :], lambda b, t: prod[:, t, b, :], mean_first, second)
                 if not second:
                     return
                 give(("prod2", j, q, r))
@@ -244,8 +252,8 @@ def tile_gaussian_nn_htanh_v_kernel(
             def interleave(n):
                 if n == 0:
                     take(("xin", g, half), "small", [P, K, T], BF16, newest=engines[0] == "g")
-                src = (tiles["x", g][:, :, cols(2 * half + n, 256)] if X_WHOLE else tiles["x", g, half][:, :, cols(n, 256)]).rearrange("p t w -> p w t")
-                copy(engines[n], tiles["xin", g, half][:, cols(n, 256), :], src)
+                src = (tiles["x", g][:, :, cols(2 * half + n, 256)] if X_WHOLE else tiles["x", g, half][:, :, cols(n, 256)]).rearrange("p t (c i) -> p c t i", i=X_RUN)
+                copy(engines[n], tiles["xin", g, half][:, cols(n, 256), :].rearrange("p (c i) t -> p c t i", i=X_RUN), src)
                 if n == 1 and not X_WHOLE:
                     give(("x", g, half))
                 if n == 1 and X_WHOLE and half == 1:
@@ -322,8 +330,8 @@ def tile_gaussian_nn_htanh_v_kernel(
                 for q in range(2):
                     if c == 0:
                         take(("w1in", j, q, xh), "small", [P, K, T], BF16)
-                    src = tiles["w1bank", i, j, q][:].rearrange("p t m -> p m t")
-                    copy(readers[q], tiles["w1in", j, q, xh][:, cols(c), :], src)
+                    src = tiles["w1bank", i, j, q][:].rearrange("p t (m i) -> p m t i", i=W_RUN)
+                    copy(readers[q], tiles["w1in", j, q, xh][:, cols(c), :].rearrange("p (m i) t -> p m t i", i=W_RUN), src)
                     give(("w1bank", i, j, q))
 
             steps = turn_steps(turn, empty, shift)
@@ -430,8 +438,12 @@ def tile_gaussian_nn_htanh_v_kernel(
             def empty():
                 dst = take(("dzin",) + key, "small", [P, K, T], BF16)
                 for s in range(2):
-                    src = tiles[("dzbank",) + key + (s,)][:].bitcast(BF16).rearrange("p u (m e) -> p e m u", e=2)
-                    nc.scalar.copy(out=dst[:, cols(s, 256), :].rearrange("p (e m) u -> p e m u", e=2), in_=src)
+                    if DZ_RUN:
+                        src = tiles[("dzbank",) + key + (s,)][:].bitcast(BF16).rearrange("p u (m i e) -> p m u i e", i=DZ_RUN, e=2)
+                        nc.scalar.copy(out=dst[:, cols(s, 256), :].rearrange("p (e m i) u -> p m u i e", e=2, i=DZ_RUN), in_=src)
+                    else:
+                        src = tiles[("dzbank",) + key + (s,)][:].bitcast(BF16).rearrange("p u (m e) -> p e m u", e=2)
+                        nc.scalar.copy(out=dst[:, cols(s, 256), :].rearrange("p (e m) u -> p e m u", e=2), in_=src)
                     give(("dzbank",) + key + (s,))
 
             steps = [(-1, READ, partial(sort, s)) for s in range(2)] if presort else []

@@ -10,7 +10,6 @@ F32 = mybir.dt.float32
 BF16 = mybir.dt.bfloat16
 U32 = mybir.dt.uint32
 U8 = mybir.dt.uint8
-I32 = mybir.dt.int32
 E4M3 = mybir.dt.float8_e4m3fn_x4
 E5M2 = mybir.dt.float8_e5m2_x4
 ALU = mybir.AluOpType
@@ -21,25 +20,23 @@ BYTES = 2 * (N * X + 2 * X * H + J * X * H + 2 * H * Y + J * H * Y + J * N * Y) 
 
 P = 128
 T = 4
-K = 512
+K = P * T
+RUN = 8
+
 EDGE = 1.0 + 3.0 / 256.0
-CENTRE = 3.0 * 2.0**22 + 1.0
+
 SMALL_SLOTS = 34
 LARGE_SLOTS = 3
 CODE_SLOTS = 30
-LEAD = 10
-AHEAD = 2
+BANKS = 8
+
+LOAD_LEAD = 10
+W2_AHEAD = 2
+W1_AHEAD = 3
 BEHIND = 3
-SORTED = 1
-WARM = 0
-P2_RUN = 2
-X_RUN = 4
-W_RUN = 1
-DZ_RUN = 0
-X_WHOLE = False
-MU_LATE = 0
-ADD_PIECES = 1
-POOL_PART = 3
+POOL_PLACES = 3
+
+PE, READ, MAKE, QUANT, POOL, DMA = range(6)
 
 
 def tile_gaussian_nn_htanh_v_kernel(
@@ -61,7 +58,7 @@ def tile_gaussian_nn_htanh_v_kernel(
             "small": list(range(SMALL_SLOTS)),
             "large": list(range(LARGE_SLOTS)),
             "code": list(range(CODE_SLOTS)),
-            "bank": list(range(8)),
+            "bank": list(range(BANKS)),
         }
         held = {}
         tiles = {}
@@ -80,33 +77,32 @@ def tile_gaussian_nn_htanh_v_kernel(
                 tiles[key] = sbuf.tile(shape, dtype, name=key[0], tag=tag, align_bytes=64)
             return tiles[key]
 
-        def give(*keys):
-            for key in keys:
-                kind, slot = held.pop(key)
-                free[kind].append(slot)
+        def give(key):
+            kind, slot = held.pop(key)
+            free[kind].append(slot)
+
+        def cols(n, width=P):
+            return slice(width * n, width * n + width)
 
         def load(key, kind, shape, dtype, src):
             nc.sync.dma_start(out=take(key, kind, shape, dtype)[:], in_=src)
 
-        sources = {}
+        def copy(engine, out, in_):
+            if engine == "s":
+                nc.scalar.copy(out=out, in_=in_)
+            elif engine == "v":
+                nc.vector.tensor_copy(out=out, in_=in_)
+            else:
+                nc.gpsimd.tensor_scalar(out=out, in0=in_, scalar1=1.0, scalar2=0.0, op0=ALU.mult, op1=ALU.add)
 
-        def quantize(key):
-            if key in tiles:
-                return
-            fmt, src_key, last_reader = sources[key]
+        def quantize(key, fmt, src_key, last_reader=True):
             words, scales = take(key, "code", [P, K], U32)
             src = tiles[src_key][:].rearrange("p c t -> p (c t)")
             nc.vector.quantize_mx(out=words[:].bitcast(fmt), scales=scales[:], in_=src)
             if last_reader:
                 give(src_key)
 
-        def quant_step(offset, key, fmt, src_key, last_reader=True):
-            sources[key] = (fmt, src_key, last_reader)
-            return (offset, QUANT, partial(quantize, key))
-
         def mx(bank, lhs_key, lhs_cols, lhs_fmt, rhs_key, rhs_cols, rhs_fmt, start, stop):
-            quantize(lhs_key)
-            quantize(rhs_key)
             lhs, rhs = tiles[lhs_key], tiles[rhs_key]
             nc.tensor.matmul_mx(
                 out=bank,
@@ -118,107 +114,70 @@ def tile_gaussian_nn_htanh_v_kernel(
                 stop=stop,
             )
 
-        def copy(engine, out, in_):
-            if engine == "s":
-                nc.scalar.copy(out=out, in_=in_)
-            elif engine == "g":
-                nc.gpsimd.tensor_scalar(out=out, in0=in_, scalar1=1.0, scalar2=0.0, op0=ALU.mult, op1=ALU.add)
-            else:
-                nc.vector.tensor_copy(out=out, in_=in_)
+        def transpose_sum(banks, mean_of, prod_of, mean_first):
+            for second in (False, True):
+                for b in range(2):
+                    for t in range(T):
+                        flags = dict(start=(t == 0 and not second), stop=(t == T - 1 and second))
+                        if mean_first != second:
+                            nc.tensor.matmul(banks[b][:, t, :], lhsT=mean_of(b, t), rhs=ident_b[:], **flags)
+                        else:
+                            nc.tensor.matmul(banks[b][:, t, :], lhsT=prod_of(b, t), rhs=ident_f[:], is_transpose=True, **flags)
 
-        def cols(n, width=P):
-            return slice(width * n, width * n + width)
 
-        def turn_sum(banks, mean_of, prod_of, mean_first, second):
-            for b in range(2):
-                for t in range(T):
-                    flags = dict(start=(t == 0 and not second), stop=(t == T - 1 and second))
-                    if mean_first != second:
-                        nc.tensor.matmul(banks[b][:, t, :], lhsT=mean_of(b, t), rhs=ident_b[:], **flags)
-                    else:
-                        nc.tensor.matmul(banks[b][:, t, :], lhsT=prod_of(b, t), rhs=ident_f[:], is_transpose=True, **flags)
-
-        def turn_steps(turn, empty, shift):
-            return [(min(shift, 0), PE, partial(turn, False)), (max(shift, 0), PE, partial(turn, True)), (max(shift, 0) + 1, READ, empty)]
-
-        PE, READ, MAKE, QUANT, POOL, DMA = range(6)
-
-        def w2_job(j, q, r, mean_first, behind=BEHIND, readers="ss", sorter="s", ahead=AHEAD, shift=0):
+        def w2_job(j, q, r, mean_first, behind=BEHIND, readers="ss"):
             split = q == 0
-            part = r if split else 0
+            piece = r if split else 0
 
-            def shared(*name):
-                return tiles[name + (q, part)][:, cols(0 if split else r, 2), :]
+            def rows(*name):
+                return tiles[name + (q, piece)][:, cols(0 if split else r, 2), :]
 
             def fetch(src, *name):
                 view = src.rearrange("(a b m) y -> a m b y", b=2 if split else 4, m=P)[r if split else q]
-                load(name + (q, part), "small", [P, 2 if split else 4, Y], BF16, view)
+                load(name + (q, piece), "small", [P, 2 if split else 4, Y], BF16, view)
 
             def release(*name):
                 if split or r == 1:
-                    give(name + (q, part))
-
-            def warm_up():
-                for n in range(WARM):
-                    if n == 0:
-                        bank = take(("warm",), "bank", [P, K], F32)
-                    nc.tensor.matmul(tiles["warm",][:], lhsT=ident_b[:], rhs=shared("sig2")[:, 0, :], start=True, stop=True)
-                if WARM:
-                    give(("warm",))
-
-            def sort_mean():
-                dst = take(("mean2", q, r), "small", [P, T, 2, P], BF16)
-                src = shared("mu2").rearrange("p b (w i t) -> p (b w) t i", t=T, i=4)
-                copy(sorter, dst[:].rearrange("p t b (w i) -> p (b w) t i", i=4), src)
-                release("mu2")
+                    give(name + (q, piece))
 
             def multiply():
                 prod = take(("prod2", j, q, r), "small", [P, T, 2, P], F32)
-                order = "p b (w i t) -> p (b w) t i"
+                walk = "p b (w i t) -> p (b w) t i"
                 nc.vector.tensor_tensor(
-                    out=prod[:].rearrange("p t b (w i) -> p (b w) t i", i=P2_RUN),
-                    in0=shared("e2", j).rearrange(order, t=T, i=P2_RUN),
-                    in1=shared("sig2").rearrange(order, t=T, i=P2_RUN),
+                    out=prod[:].rearrange("p t b (w i) -> p (b w) t i", i=2),
+                    in0=rows("e2", j).rearrange(walk, t=T, i=2),
+                    in1=rows("sig2").rearrange(walk, t=T, i=2),
                     op=ALU.mult,
                 )
                 release("e2", j)
                 if j == J - 1:
                     release("sig2")
 
-            def turn(second):
-                prod = tiles.get(("prod2", j, q, r))
-                mean = tiles["mean2", q, r] if q < SORTED else shared("mu2").rearrange("p b (w t) -> p t b w", t=T)
-                banks = [tiles["w2bank", j, q, r, b] if second else take(("w2bank", j, q, r, b), "bank", [P, T, P], F32) for b in range(2)]
-                turn_sum(banks, lambda b, t: mean[:, t, b, :], lambda b, t: prod[:, t, b, :], mean_first, second)
-                if not second:
-                    return
+            def turn():
+                prod = tiles["prod2", j, q, r]
+                mean = rows("mu2").rearrange("p b (w t) -> p t b w", t=T)
+                banks = [take(("w2bank", j, q, r, b), "bank", [P, T, P], F32) for b in range(2)]
+                transpose_sum(banks, lambda b, t: mean[:, t, b, :], lambda b, t: prod[:, t, b, :], mean_first)
                 give(("prod2", j, q, r))
-                if j == J - 1 and q < SORTED:
-                    give(("mean2", q, r))
-                if q >= SORTED and j == J - 1:
+                if j == J - 1:
                     release("mu2")
 
             def empty():
                 if r == 0:
                     take(("w2in", j, q), "small", [P, K, T], BF16)
-                dst = tiles["w2in", j, q][:].rearrange("p (u b i) t -> p u b i t", u=T, i=8)
+                dst = tiles["w2in", j, q][:].rearrange("p (u b i) t -> p u b i t", u=T, i=RUN)
                 for b in range(2):
-                    blocks = cols(2 * r + b, 4)
-                    src = tiles["w2bank", j, q, r, b][:].rearrange("p t (b u i) -> p u b i t", u=T, i=8)
-                    copy(readers[b], dst[:, :, blocks, :, :], src)
+                    src = tiles["w2bank", j, q, r, b][:].rearrange("p t (b u i) -> p u b i t", u=T, i=RUN)
+                    copy(readers[b], dst[:, :, cols(2 * r + b, 4), :, :], src)
                     give(("w2bank", j, q, r, b))
 
-            steps = [(-ahead, MAKE, multiply)] + turn_steps(turn, empty, shift)
+            steps = [(-W2_AHEAD, MAKE, multiply), (0, PE, turn), (1, READ, empty)]
             if split or r == 0:
-                if j == 0:
-                    steps.append((-LEAD - AHEAD, DMA, partial(fetch, sig_W2, "sig2")))
-                    steps.append((-LEAD - AHEAD + MU_LATE, DMA + MU_LATE, partial(fetch, mu_W2, "mu2")))
-                steps.append((-LEAD - AHEAD, DMA, partial(fetch, e_W2[j], "e2", j)))
-            if j == 0 and q < SORTED:
-                steps.append((-ahead - (1 + r if q else 0), MAKE, sort_mean))
-            if split and r == 0 and j == 0:
-                steps.append((-1, PE, warm_up))
-            return steps + ([quant_step(behind, ("w2", j, q), E4M3, ("w2in", j, q))] if r == 1 else [])
+                wanted = [(sig_W2, "sig2"), (e_W2[j], "e2", j), (mu_W2, "mu2")] if j == 0 else [(e_W2[j], "e2", j)]
+                steps += [(-LOAD_LEAD - W2_AHEAD, DMA, partial(fetch, *item)) for item in wanted]
+            if r == 1:
+                steps.append((behind, QUANT, partial(quantize, ("w2", j, q), E4M3, ("w2in", j, q))))
+            return steps
 
         def grad_job(j, g, behind=BEHIND, readers="ss"):
             def fetch():
@@ -228,44 +187,43 @@ def tile_gaussian_nn_htanh_v_kernel(
                 words = tiles["grad", j, g][:].rearrange("p t y -> p (t y)").bitcast(F32).rearrange("p (t w) -> p t w", t=T)
                 for a in range(2):
                     bank = take(("gbank", j, g, a), "bank", [P, 2, 2, P], F32)
-                    for s in range(2):
-                        for u in range(2):
-                            nc.tensor.transpose(bank[:, s, u, :], words[:, 2 * a + s, u::2], ident_f[:])
+                    for t in range(2):
+                        for s in range(2):
+                            nc.tensor.transpose(bank[:, t, s, :], words[:, 2 * a + t, s::2], ident_f[:])
                 give(("grad", j, g))
 
             def empty():
                 dst = take(("gin", j, g), "small", [P, K, T], BF16)[:].rearrange("p c t -> p (c t)").bitcast(F32)
                 for a in range(2):
-                    out = dst[:, cols(a, K)].rearrange("p (s m u) -> p s m u", s=2, u=2)
-                    copy(readers[a], out, tiles["gbank", j, g, a][:].rearrange("p s u m -> p s m u"))
+                    out = dst[:, cols(a, K)].rearrange("p (t m s) -> p t m s", t=2, s=2)
+                    copy(readers[a], out, tiles["gbank", j, g, a][:].rearrange("p t s m -> p t m s"))
                     give(("gbank", j, g, a))
 
-            return [(-LEAD - 1, DMA, fetch), (0, PE, turn), (1, READ, empty), quant_step(behind, ("g", j, g), E5M2, ("gin", j, g))]
+            quant = partial(quantize, ("g", j, g), E5M2, ("gin", j, g))
+            return [(-LOAD_LEAD - 1, DMA, fetch), (0, PE, turn), (1, READ, empty), (behind, QUANT, quant)]
 
-        def x_job(g, half, engines, behind=3):
+        def x_steps(g, half, engines):
             def fetch():
-                if X_WHOLE:
-                    load(("x", g), "large", [P, T, X], BF16, x.rearrange("(g p t) w -> g p t w", g=2, t=T)[g])
-                    return
-                load(("x", g, half), "small", [P, T, K], BF16, x.rearrange("(g p t) w -> g p t w", g=2, t=T)[g][:, :, cols(half, K)])
+                view = x.rearrange("(g p t) w -> g p t w", g=2, t=T)[g][:, :, cols(half, K)]
+                load(("x", g, half), "small", [P, T, K], BF16, view)
 
             def interleave(n):
                 if n == 0:
                     take(("xin", g, half), "small", [P, K, T], BF16, newest=engines[0] == "g")
-                src = (tiles["x", g][:, :, cols(2 * half + n, 256)] if X_WHOLE else tiles["x", g, half][:, :, cols(n, 256)]).rearrange("p t (c i) -> p c t i", i=X_RUN)
-                copy(engines[n], tiles["xin", g, half][:, cols(n, 256), :].rearrange("p (c i) t -> p c t i", i=X_RUN), src)
-                if n == 1 and not X_WHOLE:
+                src = tiles["x", g, half][:, :, cols(n, K // 2)].rearrange("p t (c i) -> p c t i", i=4)
+                copy(engines[n], tiles["xin", g, half][:, cols(n, K // 2), :].rearrange("p (c i) t -> p c t i", i=4), src)
+                if n == 1:
                     give(("x", g, half))
-                if n == 1 and X_WHOLE and half == 1:
-                    give(("x", g))
 
             steps = [(0, POOL, partial(interleave, n)) if engines[n] == "g" else (n, MAKE, partial(interleave, n)) for n in range(2)]
-            return steps + ([] if X_WHOLE and half else [(-LEAD, DMA, fetch)]) + [quant_step(behind, ("xq", g, half), E4M3, ("xin", g, half))]
+            quant = partial(quantize, ("xq", g, half), E4M3, ("xin", g, half))
+            return steps + [(-LOAD_LEAD, DMA, fetch), (BEHIND, QUANT, quant)]
 
-        def w1_job(i, j, mean_first, pool_ahead=None, readers="ss", sorter="v", behind=BEHIND, ahead=AHEAD, shift=0):
+        def w1_job(n, mean_first, pool_ahead=None, readers="ss"):
+            i, j = divmod(n, J)
             a, r = divmod(i, 2)
             xh, c = divmod(i, 4)
-            order = "p (b t i) -> p t b i"
+            sort = "p (b u i) -> p u b i"
 
             def fetch():
                 if r == 0:
@@ -275,112 +233,68 @@ def tile_gaussian_nn_htanh_v_kernel(
                     load(("mu1", a), "small", [P, 2, H], BF16, mu_W1.rearrange("(a r m) h -> a m r h", r=2, m=P)[a])
 
             def sort_mean():
-                dst = take(("mean1", a), "small", [P, 2, T, 32, 8], BF16)
-                copy(sorter, dst[:], tiles["mu1", a][:].rearrange("p r (b t i) -> p r t b i", t=T, i=8))
+                dst = take(("mean1", a), "small", [P, 2, T, 32, RUN], BF16)
+                nc.vector.tensor_copy(out=dst[:], in_=tiles["mu1", a][:].rearrange("p r (b u i) -> p r u b i", u=T, i=RUN))
                 give(("mu1", a))
 
-            def multiply(eng, part):
-                if part.start == 0:
-                    take(("prod1", i, j), "small", [P, T, 32, 8], F32, newest=pool_ahead is not None)
-                eng.tensor_tensor(
-                    out=tiles["prod1", i, j][:, part],
-                    in0=tiles["e1", i][:, j, :].rearrange(order, t=T, i=8)[:, part],
-                    in1=tiles["sig1", a][:, r, :].rearrange(order, t=T, i=8)[:, part],
+            def multiply(engine, places):
+                if places.start == 0:
+                    take(("prod1", i, j), "small", [P, T, 32, RUN], F32, newest=pool_ahead is not None)
+                engine.tensor_tensor(
+                    out=tiles["prod1", i, j][:, places],
+                    in0=tiles["e1", i][:, j, :].rearrange(sort, u=T, i=RUN)[:, places],
+                    in1=tiles["sig1", a][:, r, :].rearrange(sort, u=T, i=RUN)[:, places],
                     op=ALU.mult,
                 )
-                if r == 1 and j == J - 1 and part.stop == T:
+                if r == 1 and j == J - 1 and places.stop == T:
                     give(("sig1", a))
 
-            def turn(second):
-                prod = tiles["prod1", i, j][:].rearrange("p t (q b) i -> p t q (b i)", q=2)
-                mean = tiles["mean1", a][:, r].rearrange("p t (q b) i -> p t q (b i)", q=2)
-                banks = [tiles["w1bank", i, j, q] if second else take(("w1bank", i, j, q), "bank", [P, T, P], F32) for q in range(2)]
-                turn_sum(banks, lambda q, t: mean[:, t, q, :], lambda q, t: prod[:, t, q, :], mean_first, second)
-                if not second:
-                    return
+            def turn():
+                prod = tiles["prod1", i, j][:].rearrange("p u (q b) i -> p u q (b i)", q=2)
+                mean = tiles["mean1", a][:, r].rearrange("p u (q b) i -> p u q (b i)", q=2)
+                banks = [take(("w1bank", i, j, q), "bank", [P, T, P], F32) for q in range(2)]
+                transpose_sum(banks, lambda q, u: mean[:, u, q, :], lambda q, u: prod[:, u, q, :], mean_first)
                 give(("prod1", i, j))
                 if r == 1 and j == J - 1:
                     give(("mean1", a))
-
-            def add_mean(eng):
-                total = take(("sum1", i, j), "small", [P, 2, 256, 2], BF16)
-                pairs = "p (s e) b i -> p s (b i) e"
-                eng.tensor_tensor(out=total[:], in0=tiles["prod1", i, j][:].rearrange(pairs, e=2), in1=tiles["mean1", a][:, r].rearrange(pairs, e=2), op=ALU.add)
-                give(("prod1", i, j))
-                if r == 1 and j == J - 1:
-                    give(("mean1", a))
-
-            def turn_words():
-                words = tiles["sum1", i, j][:].rearrange("p s n e -> p (s n e)").bitcast(F32).rearrange("p (s q n) -> p s q n", s=2, q=2)
-                bank = take(("w1bank", i, j), "bank", [P, 2, 2, P], F32)
-                for q in range(2):
-                    for s in range(2):
-                        nc.tensor.transpose(bank[:, q, s, :], words[:, s, q, :], ident_f[:])
-                give(("sum1", i, j))
-
-            def empty_words():
-                for q in range(2):
-                    if c == 0:
-                        take(("w1in", j, q, xh), "small", [P, K, T], BF16)
-                    dst = tiles["w1in", j, q, xh][:, cols(c), :].rearrange("p m t -> p (m t)").bitcast(F32).rearrange("p (m s) -> p m s", s=2)
-                    copy(readers[q], dst, tiles["w1bank", i, j][:, q].rearrange("p s m -> p m s"))
-                give(("w1bank", i, j))
 
             def empty():
                 for q in range(2):
                     if c == 0:
                         take(("w1in", j, q, xh), "small", [P, K, T], BF16)
-                    src = tiles["w1bank", i, j, q][:].rearrange("p t (m i) -> p m t i", i=W_RUN)
-                    copy(readers[q], tiles["w1in", j, q, xh][:, cols(c), :].rearrange("p (m i) t -> p m t i", i=W_RUN), src)
+                    src = tiles["w1bank", i, j, q][:].rearrange("p u m -> p m u")
+                    copy(readers[q], tiles["w1in", j, q, xh][:, cols(c), :], src)
                     give(("w1bank", i, j, q))
 
-            steps = turn_steps(turn, empty, shift)
-            if mean_first is None:
-                steps = [(-1, MAKE, partial(add_mean, nc.vector)), (0, PE, turn_words), (1, READ, empty_words)]
+            steps = [(0, PE, turn), (1, READ, empty)]
             if pool_ahead is None:
-                steps.append((-ahead, MAKE, partial(multiply, nc.vector, slice(0, T))))
+                steps.append((-W1_AHEAD, MAKE, partial(multiply, nc.vector, slice(0, T))))
             else:
-                steps.append((-pool_ahead, POOL, partial(multiply, nc.gpsimd, slice(0, POOL_PART))))
-                if POOL_PART < T:
-                    steps.append((-pool_ahead + 1, MAKE, partial(multiply, nc.vector, slice(POOL_PART, T))))
+                steps.append((-pool_ahead, POOL, partial(multiply, nc.gpsimd, slice(0, POOL_PLACES))))
+                steps.append((-pool_ahead + 1, MAKE, partial(multiply, nc.vector, slice(POOL_PLACES, T))))
             if j == 0:
-                steps.append((-LEAD - AHEAD, DMA, fetch))
+                steps.append((-LOAD_LEAD - W2_AHEAD, DMA, fetch))
                 if r == 0:
-                    steps.append((-AHEAD - 1, MAKE, sort_mean))
+                    steps.append((-W1_AHEAD, MAKE, sort_mean))
             if c == 3:
-                steps += [quant_step(behind + q, ("w1", j, q, xh), E4M3, ("w1in", j, q, xh)) for q in range(2)]
+                for q in range(2):
+                    steps.append((BEHIND + q, QUANT, partial(quantize, ("w1", j, q, xh), E4M3, ("w1in", j, q, xh))))
             return steps
 
-        def dh_job(j, q, g, half, abs_ahead, markers, soon):
-            key = (j, q, g)
-            pieces = [(0, 2), (2, 2)] if markers[2] == markers[3] else [(0, 2), (2, 1), (3, 1)]
-            if markers == "llll":
-                pieces = [(0, 4)]
+        def dh_jobs(key, abs_ahead, quant_behind):
+            j, q, g = key
 
             def fetch():
-                load(("z",) + key, "large", [P, T, K], F32, z1[j].rearrange("(g p t) h -> g p t h", g=2, t=T)[g][:, :, cols(q, K)])
+                view = z1[j].rearrange("(g p t) h -> g p t h", g=2, t=T)[g][:, :, cols(q, K)]
+                load(("z",) + key, "large", [P, T, K], F32, view)
 
-            def mark_lines(n):
-                if n == 0:
-                    take(("mark",) + key + (0,), "small", [P, 16, 32, T], BF16)
-                dst = tiles[("mark",) + key + (0,)][:].rearrange("p b (c i) t -> p (b c) t i", i=4)[:, cols(n, 64)]
-                src = tiles[("z",) + key][:].rearrange("p t (c i) -> p c t i", i=4)[:, cols(n, 64)]
+            def absolute():
+                dst = take(("abs",) + key, "small", [P, K, T], BF16)[:].rearrange("p (c i) t -> p c t i", i=4)
+                src = tiles[("z",) + key][:].rearrange("p t (c i) -> p c t i", i=4)
                 nc.scalar.activation(out=dst, in_=src, func=ACT.Abs, scale=EDGE)
-                if n == 1:
-                    give(("z",) + key)
+                give(("z",) + key)
 
-            def mark(u, n):
-                src = tiles[("z",) + key][:].rearrange("p t (b h) -> p b h t", h=32)[:, :, 8 * u : 8 * (u + n), :]
-                if markers[u] == "s":
-                    dst = take(("mark",) + key + (u,), "small", [P, 16, 8 * n, T], BF16)
-                    nc.scalar.activation(out=dst[:], in_=src, func=ACT.Abs, scale=EDGE)
-                else:
-                    dst = take(("mark",) + key + (u,), "small", [P, 16, 8 * n, T], I32, newest=(u == 0))
-                    nc.gpsimd.tensor_scalar(out=dst[:], in0=src, scalar1=0.5, scalar2=CENTRE, op0=ALU.mult, op1=ALU.add)
-                if u + n == T:
-                    give(("z",) + key)
-
-            def multiply():
+            def multiply(half):
                 for u in (2 * half, 2 * half + 1):
                     bank = take(("dh",) + key + (u,), "bank", [P, T, P], F32)
                     for t in range(T):
@@ -391,101 +305,76 @@ def tile_gaussian_nn_htanh_v_kernel(
                     give(("w2", j, q))
 
             def mask():
-                take(("dz",) + key, "small", [P, K, T], BF16)
-                dz = tiles[("dz",) + key][:].rearrange("p (u b i) t -> p u b i t", u=T, i=8)
+                dz = take(("dz",) + key, "small", [P, K, T], BF16)[:].rearrange("p (u b i) t -> p u b i t", u=T, i=RUN)
+                size = tiles[("abs",) + key][:].rearrange("p (b u i) t -> p u b i t", u=T, i=RUN)
                 for u in range(T):
-                    bank = tiles[("dh",) + key + (u,)][:].rearrange("p t (b i) -> p b i t", i=8)
-                    first, n = [piece for piece in pieces if piece[0] <= u][-1]
-                    marks = tiles[("mark",) + key + (first,)][:, :, cols(u - first, 8), :]
-                    level, test = (EDGE, ALU.is_lt) if markers[u] != "g" else (CENTRE, ALU.is_equal)
-                    nc.vector.scalar_tensor_tensor(out=dz[:, u], in0=marks, scalar=level, in1=bank, op0=test, op1=ALU.mult)
+                    bank = tiles[("dh",) + key + (u,)][:].rearrange("p t (b i) -> p b i t", i=RUN)
+                    nc.vector.scalar_tensor_tensor(out=dz[:, u], in0=size[:, u], scalar=EDGE, in1=bank, op0=ALU.is_lt, op1=ALU.mult)
                     give(("dh",) + key + (u,))
-                    if u == first + n - 1:
-                        give(("mark",) + key + (first,))
+                give(("abs",) + key)
 
-            steps = [(0, PE, multiply)]
-            if half == 0:
-                steps.append((-LEAD - abs_ahead, DMA, fetch))
-                if markers == "llll":
-                    return steps + [(-abs_ahead + 1 + n, MAKE, partial(mark_lines, n)) for n in range(2)]
-                for u, n in pieces:
-                    at = (-abs_ahead, POOL) if markers[u] == "g" else (-abs_ahead + 1 + u // 2, MAKE)
-                    steps.append(at + (partial(mark, u, n),))
-                return steps
-            return steps + [(1, READ, mask), quant_step(soon, ("dzn",) + key, E5M2, ("dz",) + key, False)]
+            quant = partial(quantize, ("dzn",) + key, E5M2, ("dz",) + key, last_reader=False)
+            first = [(0, PE, partial(multiply, 0)), (-LOAD_LEAD - abs_ahead - 1, DMA, fetch), (-abs_ahead, MAKE, absolute)]
+            second = [(0, PE, partial(multiply, 1)), (1, READ, mask), (quant_behind, QUANT, quant)]
+            return first, second
 
-        def dzt_job(j, q, g, behind, presort):
-            key = (j, q, g)
-
-            def pairs():
-                return tiles[("dz",) + key][:].rearrange("p c t -> p (c t)").bitcast(F32).rearrange("p (u m s) -> p s u m", u=T, s=2)
-
-            def sort(s):
-                if s == 0:
-                    take(("dzw",) + key, "small", [P, 2, T, P], F32)
-                copy(presort, tiles[("dzw",) + key][:, s], pairs()[:, s])
-
+        def dz_job(key, behind):
             def turn():
-                words = tiles[("dzw",) + key][:] if presort else pairs()
+                words = tiles[("dz",) + key][:].rearrange("p c t -> p (c t)").bitcast(F32).rearrange("p (u m s) -> p s u m", u=T, s=2)
                 for s in range(2):
                     bank = take(("dzbank",) + key + (s,), "bank", [P, T, P], F32)
                     for u in range(T):
                         nc.tensor.transpose(bank[:, u, :], words[:, s, u, :], ident_f[:])
                 give(("dz",) + key)
-                if presort:
-                    give(("dzw",) + key)
 
             def empty():
                 dst = take(("dzin",) + key, "small", [P, K, T], BF16)
                 for s in range(2):
-                    if DZ_RUN:
-                        src = tiles[("dzbank",) + key + (s,)][:].bitcast(BF16).rearrange("p u (m i e) -> p m u i e", i=DZ_RUN, e=2)
-                        nc.scalar.copy(out=dst[:, cols(s, 256), :].rearrange("p (e m i) u -> p m u i e", e=2, i=DZ_RUN), in_=src)
-                    else:
-                        src = tiles[("dzbank",) + key + (s,)][:].bitcast(BF16).rearrange("p u (m e) -> p e m u", e=2)
-                        nc.scalar.copy(out=dst[:, cols(s, 256), :].rearrange("p (e m) u -> p e m u", e=2), in_=src)
+                    src = tiles[("dzbank",) + key + (s,)][:].bitcast(BF16).rearrange("p u (m e) -> p e m u", e=2)
+                    nc.scalar.copy(out=dst[:, cols(s, K // 2), :].rearrange("p (e m) u -> p e m u", e=2), in_=src)
                     give(("dzbank",) + key + (s,))
 
-            steps = [(-1, READ, partial(sort, s)) for s in range(2)] if presort else []
-            return steps + [(0, PE, turn), (1, READ, empty), quant_step(behind, ("dzh",) + key, E5M2, ("dzin",) + key)]
+            quant = partial(quantize, ("dzh",) + key, E5M2, ("dzin",) + key)
+            return [(0, PE, turn), (1, READ, empty), (behind, QUANT, quant)]
 
-        def dx_job(g, xh, t, width=2, passes=range(4), reader="s", queue=nc.sync):
-            pair = (g, xh, t // width)
+        def dx_job(g, xh, t, together=1, piece=0, pieces=1, reader="s"):
+            width = K // pieces
+            bank_key = ("dx", g, xh, t, piece)
+            out_key = ("out0", g, xh, t // together, piece)
 
             def multiply():
-                if 0 in passes:
-                    take(("dx", g, xh, t), "bank", [P, K], F32)
-                bank = tiles["dx", g, xh, t]
-                for k in passes:
-                    q, j = divmod(k, 2)
-                    mx(bank[:], ("dzh", j, q, g), cols(t), E5M2, ("w1", j, q, xh), cols(0, K), E4M3, k == 0, k == 3)
-                    if t == T - 1 and xh == 1:
+                bank = take(bank_key, "bank", [P, width], F32)
+                for k in range(2 * J):
+                    q, j = divmod(k, J)
+                    mx(bank[:], ("dzh", j, q, g), cols(t), E5M2, ("w1", j, q, xh), cols(piece, width), E4M3, k == 0, k == 2 * J - 1)
+                    if t == T - 1 and xh == 1 and g == 0:
                         give(("dzh", j, q, g))
-                    if t == T - 1 and g == 1:
+                    if t == T - 1 and xh == 0 and g == 1:
                         give(("w1", j, q, xh))
 
             def empty():
-                if t % width == 0:
-                    take(("out0",) + pair, "small", [P, width, K], F32)
-                copy(reader, tiles[("out0",) + pair][:, t % width, :], tiles["dx", g, xh, t][:])
-                give(("dx", g, xh, t))
+                if t % together == 0:
+                    take(out_key, "small", [P, together, width], F32)
+                copy(reader, tiles[out_key][:, t % together, :], tiles[bank_key][:])
+                give(bank_key)
 
             def store():
-                dst = out_0.rearrange("(g p t) w -> g p t w", g=2, t=T)[g][:, cols(t // width, width), cols(xh, K)]
-                queue.dma_start(out=dst, in_=tiles[("out0",) + pair][:])
-                give(("out0",) + pair)
+                view = out_0.rearrange("(g p t) w -> g p t w", g=2, t=T)[g]
+                nc.sync.dma_start(out=view[:, cols(t // together, together), cols(pieces * xh + piece, width)], in_=tiles[out_key][:])
+                give(out_key)
 
-            if 3 not in passes:
-                return [(0, PE, multiply)]
-            return [(0, PE, multiply), (1, READ, empty)] + ([(1, DMA, store)] if t % width == width - 1 else [])
+            steps = [(0, PE, multiply), (1, READ, empty)]
+            return steps + ([(1, DMA, store)] if t % together == together - 1 else [])
 
-        def dw_job(q, items, engine, store_behind=1):
+        def dw_job(q, items, adders, store_behind):
+            natural = "p (b u i) -> p b u i"
+
             def multiply():
                 for i, j in items:
                     bank = take(("dw", q, i, j), "bank", [P, K], F32)
                     for g in range(2):
                         mx(bank[:], ("xq", g, i // 4), cols(i % 4), E4M3, ("dzn", j, q, g), cols(0, K), E5M2, g == 0, g == 1)
-                        if i == 7:
+                        if i == X // P - 1:
                             give(("dzn", j, q, g))
 
             def weigh():
@@ -493,9 +382,9 @@ def tile_gaussian_nn_htanh_v_kernel(
                     if i % 2 == 0:
                         take(("part", q, i // 2, j), "small", [P, 2, K], F32)
                     nc.vector.tensor_tensor(
-                        out=tiles["part", q, i // 2, j][:, i % 2, :].rearrange("p (b u i) -> p b u i", u=T, i=8),
-                        in0=tiles["e1", i][:, j, cols(q, K)].rearrange("p (b u i) -> p b u i", u=T, i=8),
-                        in1=tiles["dw", q, i, j][:].rearrange("p (u b i) -> p b u i", u=T, i=8),
+                        out=tiles["part", q, i // 2, j][:, i % 2, :].rearrange(natural, u=T, i=RUN),
+                        in0=tiles["e1", i][:, j, cols(q, K)].rearrange(natural, u=T, i=RUN),
+                        in1=tiles["dw", q, i, j][:].rearrange("p (u b i) -> p b u i", u=T, i=RUN),
                         op=ALU.mult,
                     )
                     give(("dw", q, i, j))
@@ -503,90 +392,82 @@ def tile_gaussian_nn_htanh_v_kernel(
                         give(("e1", i))
 
             def add(i):
-                first, second = tiles["part", q, i // 2, 0][:, i % 2, :], tiles["part", q, i // 2, 1][:, i % 2, :]
-                eng = nc.gpsimd if engine[i % len(engine)] == "g" else nc.vector
-                pieces = ADD_PIECES if eng is nc.gpsimd else 1
-                for n in range(pieces):
-                    part = cols(n, K // pieces)
-                    eng.tensor_tensor(out=first[:, part], in0=first[:, part], in1=second[:, part], op=ALU.add)
+                total = tiles["part", q, i // 2, 0][:, i % 2, :]
+                engine = nc.gpsimd if adders[i] == "g" else nc.vector
+                engine.tensor_tensor(out=total, in0=total, in1=tiles["part", q, i // 2, 1][:, i % 2, :], op=ALU.add)
                 if i % 2 == 1:
                     give(("part", q, i // 2, 1))
 
             def store(i):
-                dst = out_1.rearrange("(a r m) h -> a m r h", r=2, m=P)[i // 2][:, :, cols(q, K)]
-                nc.sync.dma_start(out=dst, in_=tiles["part", q, i // 2, 0][:])
+                view = out_1.rearrange("(a r m) h -> a m r h", r=2, m=P)[i // 2][:, :, cols(q, K)]
+                nc.sync.dma_start(out=view, in_=tiles["part", q, i // 2, 0][:])
                 give(("part", q, i // 2, 0))
 
             done = [i for i, j in items if j == J - 1]
-            steps = [(0, PE, multiply), (1, READ, weigh), (1, MAKE, lambda: [add(i) for i in done])]
-            return steps + [(store_behind, DMA, lambda: [store(i) for i in done if i % 2 == 1])]
-
-        def dx_last(g, xh, t, part, reader):
-            key = ("dx", g, xh, t, part)
-
-            def multiply():
-                bank = take(key, "bank", [P, K // 2], F32)
-                for k in range(4):
-                    q, j = divmod(k, 2)
-                    mx(bank[:], ("dzh", j, q, g), cols(t), E5M2, ("w1", j, q, xh), cols(part, K // 2), E4M3, k == 0, k == 3)
-
-            def empty():
-                copy(reader, take(("out0",) + key, "small", [P, K // 2], F32)[:], tiles[key][:])
-                give(key)
-
-            def store():
-                dst = out_0.rearrange("(g p t) w -> g p t w", g=2, t=T)[g][:, t, cols(2 * xh + part, K // 2)]
-                (nc.scalar if reader == "s" else nc.sync).dma_start(out=dst, in_=tiles[("out0",) + key][:])
-                give(("out0",) + key)
-
-            return [(0, PE, multiply), (1, READ, empty), (1, DMA, store)]
-
-        def dx_jobs(g, xh, width=2, passes=range(4), queue=nc.sync):
-            return [dx_job(g, xh, t, width, passes, "s", queue) for t in range(T)]
-
-        def dw_jobs(q, j, engine):
-            return [dw_job(q, [(i, j), (i + 1, j)], engine) for i in range(0, 8, 2)]
+            steps = [(0, PE, multiply), (1, READ, weigh)] + [(1, MAKE, partial(add, i)) for i in done]
+            return steps + [(store_behind, DMA, partial(store, i)) for i in done if i % 2 == 1]
 
         jobs = []
         starts = []
 
-        def unit(key, markers, early, late, behind=BEHIND, beside=(), soon=2, ahead=None, presort=None):
-            ahead = ahead or (len(jobs) - starts[-1] - 1 if starts else 3)
+        def unit(key, early, late, beside=(), quant_behind=2, last=False):
+            abs_ahead = len(jobs) - starts[-1] - 2 if starts else 2
             starts.append(len(jobs))
-            jobs.extend([dh_job(*key, 0, ahead, markers, soon), dh_job(*key, 1, ahead, markers, soon) + list(beside)] + early + [dzt_job(*key, behind, presort)] + late)
+            first, second = dh_jobs(key, abs_ahead, quant_behind)
+            jobs.extend([first, second + list(beside)] + early + [dz_job(key, 2 if last else len(late) + 2)] + late)
 
         def weave(first, second):
-            jobs = []
+            woven = []
             for n in range(max(len(first), len(second))):
-                jobs += first[n : n + 1] + second[n : n + 1]
-            return jobs
+                woven += first[n : n + 1] + second[n : n + 1]
+            return woven
 
-        order = [(j, q, g) for g in range(2) for q in range(2) for j in range(J)]
-        first = dx_jobs(0, 0) + dx_jobs(0, 1)
-        first = dx_jobs(0, 0) + dx_jobs(0, 1)
-        def w1(n, mean_first, shift=0, pool_ahead=None, readers="ss", behind=BEHIND, ahead=3, sorter="v"):
-            return w1_job(n // 2, n % 2, mean_first, pool_ahead, readers, sorter, behind, ahead, shift)
-
-        jobs.extend([w2_job(0, 0, 0, False), w2_job(0, 0, 1, True, 2), grad_job(0, 0, 1, "vv"), w2_job(1, 0, 0, False)])
-        unit(order[0], "ssss", [w2_job(1, 0, 1, True), grad_job(1, 0)], [w2_job(0, 1, 0, False), w2_job(0, 1, 1, True), w2_job(1, 1, 0, False)], 5)
-        unit(order[1], "llll", [w2_job(1, 1, 1, True), w1(0, False), w1(1, True, 0, 3)], [w1(2, False)], 3, ahead=4)
-        unit(order[2], "llll", [w1(3, True), w1(4, False), w1(5, True, 0, 3, "vs")], [w1(6, False), w1(7, False)], 4)
-        unit(order[3], "llll", [w1(8, True), grad_job(0, 1, 4), w1(9, True)], [w1(10, False) + x_job(0, 1, "vv"), w1(11, True), grad_job(1, 1, 5)], 5, x_job(0, 0, "gv", 5))
-        dx = dx_jobs(0, 0)
-        unit(order[4], "llll", [dx[0], dx[1], w1(12, True)], [w1(13, False), dx[2] + x_job(1, 1, "vv", 3), dx[3]], 5, x_job(1, 0, "gv", 5))
-        dw = dw_jobs(0, 0, "g")
-        unit(order[5], "llll", [dw[0], dw[1], w1(14, True, 0, 3)], [w1(15, False, 0, 3), dw[2], dw[3]], 5, soon=3)
-        dx = dx_jobs(0, 1)
-        dw = dw_jobs(0, 1, "g")
-        unit(order[6], "llll", dw[:2] + dx[:1], weave(dw[2:], dx[1:]), 3, soon=1)
-        both = [(i, 0) for i in range(4)] + [(i, 1) for i in range(4)] + [(i, j) for i in range(4, 8) for j in range(J)]
-        dw = [dw_job(1, both[n : n + 2], "vgvggggg", 3) for n in range(0, 16, 2)]
-        unit(order[7], "llll", dw[:2], dw[2:6], 2, soon=1)
-        jobs.extend(weave(dx_jobs(1, 0, 1) + dx_jobs(1, 1, 1)[:3] + [dx_last(1, 1, 3, 0, "s"), dx_last(1, 1, 3, 1, "v")], dw[6:]))
+        jobs.extend([w2_job(0, 0, 0, False), w2_job(0, 0, 1, True, behind=2), grad_job(0, 0, behind=1, readers="vv"), w2_job(1, 0, 0, False)])
+        unit(
+            (0, 0, 0),
+            [w2_job(1, 0, 1, True, readers="vv"), grad_job(1, 0)],
+            [w2_job(0, 1, 0, False), w2_job(0, 1, 1, True), w2_job(1, 1, 0, False)],
+        )
+        unit((1, 0, 0), [w2_job(1, 1, 1, True), w1_job(0, False), w1_job(1, True)], [w1_job(2, False, pool_ahead=5)])
+        unit(
+            (0, 1, 0),
+            [w1_job(3, True), w1_job(4, False), w1_job(5, True, pool_ahead=3, readers="vs")],
+            [w1_job(6, False), w1_job(7, False)],
+        )
+        unit(
+            (1, 1, 0),
+            [w1_job(8, True), grad_job(0, 1, behind=BEHIND + 1), w1_job(9, True)],
+            [w1_job(10, False) + x_steps(0, 1, "vv"), w1_job(11, True), grad_job(1, 1, behind=BEHIND + 1)],
+            beside=x_steps(0, 0, "gv"),
+        )
+        dx = [dx_job(0, 0, t, together=2) for t in range(T)]
+        unit(
+            (0, 0, 1),
+            [dx[0], dx[1], w1_job(12, True)],
+            [w1_job(13, False), dx[2] + x_steps(1, 1, "vv"), dx[3]],
+            beside=x_steps(1, 0, "gv"),
+        )
+        rows = X // P
+        dw = [dw_job(0, [(i, 0), (i + 1, 0)], "", 1) for i in range(0, rows, 2)]
+        unit(
+            (1, 0, 1),
+            [dw[0], dw[1], w1_job(14, True, pool_ahead=3)],
+            [w1_job(15, False, pool_ahead=3), dw[2], dw[3]],
+            quant_behind=3,
+        )
+        dx = [dx_job(0, 1, t, together=2) for t in range(T)]
+        dw = [dw_job(0, [(i, 1), (i + 1, 1)], "g" * rows, 1) for i in range(0, rows, 2)]
+        unit((0, 1, 1), dw[:2] + dx[:1], weave(dw[2:], dx[1:]))
+        items = [(i, j) for j in range(J) for i in range(rows // 2)] + [(i, j) for i in range(rows // 2, rows) for j in range(J)]
+        dw = [dw_job(1, items[n : n + 2], "vgvg" + "gg" + "vv", BEHIND) for n in range(0, len(items), 2)]
+        unit((1, 1, 1), dw[:2], dw[2:6], last=True)
+        dx = [dx_job(1, xh, t) for xh in range(2) for t in range(T)][:-1]
+        dx += [dx_job(1, 1, T - 1, piece=n, pieces=2, reader="sv"[n]) for n in range(2)]
+        jobs.extend(weave(dx, dw[6:]))
 
         steps = []
-        for tick in range(len(jobs)):
-            for offset, rank, step in jobs[tick]:
-                steps.append((tick + offset, rank, len(steps), step))
+        for place in range(len(jobs)):
+            for offset, rank, step in jobs[place]:
+                steps.append((place + offset, rank, len(steps), step))
         for at, rank, n, step in sorted(steps):
             step()

@@ -140,6 +140,12 @@ def tile_gaussian_nn_htanh_v_kernel(
                 if split or r == 1:
                     give(name + (q, piece))
 
+            def sort_mean():
+                dst = take(("mean2", r), "small", [P, T, 2, P], BF16)
+                src = rows("mu2").rearrange("p b (w i t) -> p (b w) t i", t=T, i=4)
+                nc.scalar.copy(out=dst[:].rearrange("p t b (w i) -> p (b w) t i", i=4), in_=src)
+                release("mu2")
+
             def multiply():
                 prod = take(("prod2", j, q, r), "small", [P, T, 2, P], F32)
                 walk = "p b (w i t) -> p (b w) t i"
@@ -155,11 +161,13 @@ def tile_gaussian_nn_htanh_v_kernel(
 
             def turn():
                 prod = tiles["prod2", j, q, r]
-                mean = rows("mu2").rearrange("p b (w t) -> p t b w", t=T)
+                mean = tiles["mean2", r] if split else rows("mu2").rearrange("p b (w t) -> p t b w", t=T)
                 banks = [take(("w2bank", j, q, r, b), "bank", [P, T, P], F32) for b in range(2)]
                 transpose_sum(banks, lambda b, t: mean[:, t, b, :], lambda b, t: prod[:, t, b, :], mean_first)
                 give(("prod2", j, q, r))
-                if j == J - 1:
+                if j == J - 1 and split:
+                    give(("mean2", r))
+                if j == J - 1 and not split:
                     release("mu2")
 
             def empty():
@@ -175,6 +183,8 @@ def tile_gaussian_nn_htanh_v_kernel(
             if split or r == 0:
                 wanted = [(sig_W2, "sig2"), (e_W2[j], "e2", j), (mu_W2, "mu2")] if j == 0 else [(e_W2[j], "e2", j)]
                 steps += [(-LOAD_LEAD - W2_AHEAD, DMA, partial(fetch, *item)) for item in wanted]
+            if split and j == 0:
+                steps.append((-W2_AHEAD, MAKE, sort_mean))
             if r == 1:
                 steps.append((behind, QUANT, partial(quantize, ("w2", j, q), E4M3, ("w2in", j, q))))
             return steps
@@ -288,11 +298,14 @@ def tile_gaussian_nn_htanh_v_kernel(
                 view = z1[j].rearrange("(g p t) h -> g p t h", g=2, t=T)[g][:, :, cols(q, K)]
                 load(("z",) + key, "large", [P, T, K], F32, view)
 
-            def absolute():
-                dst = take(("abs",) + key, "small", [P, K, T], BF16)[:].rearrange("p (c i) t -> p c t i", i=4)
-                src = tiles[("z",) + key][:].rearrange("p t (c i) -> p c t i", i=4)
+            def absolute(n):
+                if n == 0:
+                    take(("abs",) + key, "small", [P, K, T], BF16)
+                dst = tiles[("abs",) + key][:, cols(n, K // 2), :].rearrange("p (c i) t -> p c t i", i=4)
+                src = tiles[("z",) + key][:, :, cols(n, K // 2)].rearrange("p t (c i) -> p c t i", i=4)
                 nc.scalar.activation(out=dst, in_=src, func=ACT.Abs, scale=EDGE)
-                give(("z",) + key)
+                if n == 1:
+                    give(("z",) + key)
 
             def multiply(half):
                 for u in (2 * half, 2 * half + 1):
@@ -314,7 +327,8 @@ def tile_gaussian_nn_htanh_v_kernel(
                 give(("abs",) + key)
 
             quant = partial(quantize, ("dzn",) + key, E5M2, ("dz",) + key, last_reader=False)
-            first = [(0, PE, partial(multiply, 0)), (-LOAD_LEAD - abs_ahead - 1, DMA, fetch), (-abs_ahead, MAKE, absolute)]
+            first = [(0, PE, partial(multiply, 0)), (-LOAD_LEAD - abs_ahead - 1, DMA, fetch)]
+            first += [(n - abs_ahead, MAKE, partial(absolute, n)) for n in range(2)]
             second = [(0, PE, partial(multiply, 1)), (1, READ, mask), (quant_behind, QUANT, quant)]
             return first, second
 
@@ -411,7 +425,7 @@ def tile_gaussian_nn_htanh_v_kernel(
         starts = []
 
         def unit(key, early, late, beside=(), quant_behind=2, last=False):
-            abs_ahead = len(jobs) - starts[-1] - 2 if starts else 2
+            abs_ahead = len(jobs) - starts[-1] - 2 if len(starts) > 1 else 2 + len(starts)
             starts.append(len(jobs))
             first, second = dh_jobs(key, abs_ahead, quant_behind)
             jobs.extend([first, second + list(beside)] + early + [dz_job(key, 2 if last else len(late) + 2)] + late)
@@ -425,10 +439,10 @@ def tile_gaussian_nn_htanh_v_kernel(
         jobs.extend([w2_job(0, 0, 0, False), w2_job(0, 0, 1, True, behind=2), grad_job(0, 0, behind=1, readers="vv"), w2_job(1, 0, 0, False)])
         unit(
             (0, 0, 0),
-            [w2_job(1, 0, 1, True, readers="vv"), grad_job(1, 0)],
+            [w2_job(1, 0, 1, True), grad_job(1, 0)],
             [w2_job(0, 1, 0, False), w2_job(0, 1, 1, True), w2_job(1, 1, 0, False)],
         )
-        unit((1, 0, 0), [w2_job(1, 1, 1, True), w1_job(0, False), w1_job(1, True)], [w1_job(2, False, pool_ahead=5)])
+        unit((1, 0, 0), [w2_job(1, 1, 1, True), w1_job(0, False), w1_job(1, True, pool_ahead=3)], [w1_job(2, False)])
         unit(
             (0, 1, 0),
             [w1_job(3, True), w1_job(4, False), w1_job(5, True, pool_ahead=3, readers="vs")],
@@ -459,7 +473,7 @@ def tile_gaussian_nn_htanh_v_kernel(
         dw = [dw_job(0, [(i, 1), (i + 1, 1)], "g" * rows, 1) for i in range(0, rows, 2)]
         unit((0, 1, 1), dw[:2] + dx[:1], weave(dw[2:], dx[1:]))
         items = [(i, j) for j in range(J) for i in range(rows // 2)] + [(i, j) for i in range(rows // 2, rows) for j in range(J)]
-        dw = [dw_job(1, items[n : n + 2], "vgvg" + "gg" + "vv", BEHIND) for n in range(0, len(items), 2)]
+        dw = [dw_job(1, items[n : n + 2], "vgvg" + "gggg", BEHIND) for n in range(0, len(items), 2)]
         unit((1, 1, 1), dw[:2], dw[2:6], last=True)
         dx = [dx_job(1, xh, t) for xh in range(2) for t in range(T)][:-1]
         dx += [dx_job(1, 1, T - 1, piece=n, pieces=2, reader="sv"[n]) for n in range(2)]

@@ -25,18 +25,9 @@ RUN = 8
 
 EDGE = 1.0 + 3.0 / 256.0
 
-SMALL_SLOTS = 34
-LARGE_SLOTS = 3
-CODE_SLOTS = 30
-BANKS = 8
+UNITS = [(j, q, g) for g in range(2) for q in range(2) for j in range(J)]
 
-LOAD_LEAD = 10
-W2_AHEAD = 2
-W1_AHEAD = 3
-BEHIND = 3
-POOL_PLACES = 3
-
-PE, READ, MAKE, QUANT, POOL, DMA = range(6)
+SLOTS = {"load": 14, "work": 16, "z": 3, "w1in": 2, "code": 22, "wide": 4, "bank": 8}
 
 
 def tile_gaussian_nn_htanh_v_kernel(
@@ -54,53 +45,36 @@ def tile_gaussian_nn_htanh_v_kernel(
         nc.vector.tensor_copy(out=ident_b[:], in_=ident_f[:])
         ctx.enter_context(tc.manual_schedule())
 
-        free = {
-            "small": list(range(SMALL_SLOTS)),
-            "large": list(range(LARGE_SLOTS)),
-            "code": list(range(CODE_SLOTS)),
-            "bank": list(range(BANKS)),
-        }
-        held = {}
         tiles = {}
+        specs = {}
+        steps = {}
 
-        def take(key, kind, shape, dtype, newest=False):
-            slot = free[kind].pop(-1 if newest else 0)
-            held[key] = (kind, slot)
-            tag = "%s%d" % (kind, slot)
-            if kind == "bank":
-                tiles[key] = psum.tile(shape, dtype, name=key[0], tag=tag)
-            elif kind == "code":
-                words = sbuf.tile(shape, U32, name=key[0], tag=tag, align_bytes=64)
-                scales = sbuf.tile(shape, U8, name=key[0] + "_s", tag=tag + "_s", align_bytes=64)
-                tiles[key] = (words, scales)
-            else:
-                tiles[key] = sbuf.tile(shape, dtype, name=key[0], tag=tag, align_bytes=64)
-            return tiles[key]
-
-        def give(key):
-            kind, slot = held.pop(key)
-            free[kind].append(slot)
+        def step(name, reads, writes, work):
+            steps[name] = (reads, writes, work)
 
         def cols(n, width=P):
             return slice(width * n, width * n + width)
 
-        def load(key, kind, shape, dtype, src):
-            nc.sync.dma_start(out=take(key, kind, shape, dtype)[:], in_=src)
-
         def copy(engine, out, in_):
-            if engine == "s":
+            if engine is nc.scalar:
                 nc.scalar.copy(out=out, in_=in_)
-            elif engine == "v":
+            elif engine is nc.vector:
                 nc.vector.tensor_copy(out=out, in_=in_)
             else:
                 nc.gpsimd.tensor_scalar(out=out, in0=in_, scalar1=1.0, scalar2=0.0, op0=ALU.mult, op1=ALU.add)
 
-        def quantize(key, fmt, src_key, last_reader=True):
-            words, scales = take(key, "code", [P, K], U32)
-            src = tiles[src_key][:].rearrange("p c t -> p (c t)")
-            nc.vector.quantize_mx(out=words[:].bitcast(fmt), scales=scales[:], in_=src)
-            if last_reader:
-                give(src_key)
+        def load(key, kind, shape, dtype, src):
+            specs[key] = (kind, shape, dtype)
+            step(("load",) + key, [], [key], lambda engine: engine.dma_start(out=tiles[key][:], in_=src))
+
+        def quantize(key, fmt, src_key, kind="code"):
+            def work(engine):
+                words, scales = tiles[key]
+                src = tiles[src_key][:].rearrange("p c t -> p (c t)")
+                engine.quantize_mx(out=words[:].bitcast(fmt), scales=scales[:], in_=src)
+
+            specs[key] = (kind, [P, specs[src_key][1][1]], U32)
+            step(("quant",) + key, [src_key], [key], work)
 
         def mx(bank, lhs_key, lhs_cols, lhs_fmt, rhs_key, rhs_cols, rhs_fmt, start, stop):
             lhs, rhs = tiles[lhs_key], tiles[rhs_key]
@@ -114,374 +88,441 @@ def tile_gaussian_nn_htanh_v_kernel(
                 stop=stop,
             )
 
-        def transpose_sum(banks, mean_of, prod_of, mean_first):
-            for second in (False, True):
-                for b in range(2):
-                    for t in range(T):
-                        flags = dict(start=(t == 0 and not second), stop=(t == T - 1 and second))
-                        if mean_first != second:
-                            nc.tensor.matmul(banks[b][:, t, :], lhsT=mean_of(b, t), rhs=ident_b[:], **flags)
-                        else:
-                            nc.tensor.matmul(banks[b][:, t, :], lhsT=prod_of(b, t), rhs=ident_f[:], is_transpose=True, **flags)
+        def turn_part(banks, block_of, is_mean, first):
+            for b in range(2):
+                for t in range(T):
+                    flags = dict(start=(first and t == 0), stop=(not first and t == T - 1))
+                    if is_mean:
+                        nc.tensor.matmul(tiles[banks[b]][:, t, :], lhsT=block_of(b, t), rhs=ident_b[:], **flags)
+                    else:
+                        nc.tensor.matmul(tiles[banks[b]][:, t, :], lhsT=block_of(b, t), rhs=ident_f[:], is_transpose=True, **flags)
 
+        def banks_for(key, count, shape):
+            names = [key + (b,) for b in range(count)]
+            for name in names:
+                specs[name] = ("bank", shape, F32)
+            return names
 
-        def w2_job(j, q, r, mean_first, behind=BEHIND, readers="ss"):
-            split = q == 0
-            piece = r if split else 0
+        def w2_rows(a):
+            q, r = divmod(a, 2)
+            for name, src in (("sig2", sig_W2), ("mu2", mu_W2)):
+                load((name, a), "load", [P, 2, Y], BF16, src.rearrange("(a b m) y -> a m b y", b=2, m=P)[a])
+            specs["mean2", a] = ("work", [P, T, 2, P], BF16)
 
-            def rows(*name):
-                return tiles[name + (q, piece)][:, cols(0 if split else r, 2), :]
+            def sort_mean(engine):
+                src = tiles["mu2", a][:].rearrange("p b (w i t) -> p (b w) t i", t=T, i=4)
+                copy(engine, tiles["mean2", a][:].rearrange("p t b (w i) -> p (b w) t i", i=4), src)
 
-            def fetch(src, *name):
-                view = src.rearrange("(a b m) y -> a m b y", b=2 if split else 4, m=P)[r if split else q]
-                load(name + (q, piece), "small", [P, 2 if split else 4, Y], BF16, view)
+            step(("sort2", a), [("mu2", a)], [("mean2", a)], sort_mean)
+            for j in range(J):
+                w2_sample(j, a, q, r)
 
-            def release(*name):
-                if split or r == 1:
-                    give(name + (q, piece))
+        def w2_sample(j, a, q, r):
+            load(("e2", j, a), "load", [P, 2, Y], BF16, e_W2[j].rearrange("(a b m) y -> a m b y", b=2, m=P)[a])
+            specs["prod2", j, a] = ("work", [P, T, 2, P], F32)
+            specs["w2in", j, q] = ("work", [P, K, T], BF16)
+            banks = banks_for(("w2bank", j, a), 2, [P, T, P])
 
-            def sort_mean():
-                dst = take(("mean2", r), "small", [P, T, 2, P], BF16)
-                src = rows("mu2").rearrange("p b (w i t) -> p (b w) t i", t=T, i=4)
-                nc.scalar.copy(out=dst[:].rearrange("p t b (w i) -> p (b w) t i", i=4), in_=src)
-                release("mu2")
-
-            def multiply():
-                prod = take(("prod2", j, q, r), "small", [P, T, 2, P], F32)
+            def multiply(engine):
                 walk = "p b (w i t) -> p (b w) t i"
-                nc.vector.tensor_tensor(
-                    out=prod[:].rearrange("p t b (w i) -> p (b w) t i", i=2),
-                    in0=rows("e2", j).rearrange(walk, t=T, i=2),
-                    in1=rows("sig2").rearrange(walk, t=T, i=2),
+                engine.tensor_tensor(
+                    out=tiles["prod2", j, a][:].rearrange("p t b (w i) -> p (b w) t i", i=2),
+                    in0=tiles["e2", j, a][:].rearrange(walk, t=T, i=2),
+                    in1=tiles["sig2", a][:].rearrange(walk, t=T, i=2),
                     op=ALU.mult,
                 )
-                release("e2", j)
-                if j == J - 1:
-                    release("sig2")
 
-            def turn():
-                prod = tiles["prod2", j, q, r]
-                mean = tiles["mean2", r] if split else rows("mu2").rearrange("p b (w t) -> p t b w", t=T)
-                banks = [take(("w2bank", j, q, r, b), "bank", [P, T, P], F32) for b in range(2)]
-                transpose_sum(banks, lambda b, t: mean[:, t, b, :], lambda b, t: prod[:, t, b, :], mean_first)
-                give(("prod2", j, q, r))
-                if j == J - 1 and split:
-                    give(("mean2", r))
-                if j == J - 1 and not split:
-                    release("mu2")
+            def turn(source, first, engine):
+                block = tiles[source][:].rearrange("p b (w t) -> p t b w", t=T) if source[0] == "mu2" else tiles[source]
+                turn_part(banks, lambda b, t: block[:, t, b, :], source[0] != "prod2", first)
 
-            def empty():
-                if r == 0:
-                    take(("w2in", j, q), "small", [P, K, T], BF16)
+            def empty(b, engine):
                 dst = tiles["w2in", j, q][:].rearrange("p (u b i) t -> p u b i t", u=T, i=RUN)
-                for b in range(2):
-                    src = tiles["w2bank", j, q, r, b][:].rearrange("p t (b u i) -> p u b i t", u=T, i=RUN)
-                    copy(readers[b], dst[:, :, cols(2 * r + b, 4), :, :], src)
-                    give(("w2bank", j, q, r, b))
+                src = tiles[banks[b]][:].rearrange("p t (b u i) -> p u b i t", u=T, i=RUN)
+                copy(engine, dst[:, :, cols(2 * r + b, 4), :, :], src)
 
-            steps = [(-W2_AHEAD, MAKE, multiply), (0, PE, turn), (1, READ, empty)]
-            if split or r == 0:
-                wanted = [(sig_W2, "sig2"), (e_W2[j], "e2", j), (mu_W2, "mu2")] if j == 0 else [(e_W2[j], "e2", j)]
-                steps += [(-LOAD_LEAD - W2_AHEAD, DMA, partial(fetch, *item)) for item in wanted]
-            if split and j == 0:
-                steps.append((-W2_AHEAD, MAKE, sort_mean))
-            if r == 1:
-                steps.append((behind, QUANT, partial(quantize, ("w2", j, q), E4M3, ("w2in", j, q))))
-            return steps
+            step(("mul2", j, a), [("e2", j, a), ("sig2", a)], [("prod2", j, a)], multiply)
+            for first in (False, True):
+                for name, source in (("turn2", ("prod2", j, a)), ("mean2", ("mean2", a)), ("raw2", ("mu2", a))):
+                    step((name, j, a, first), [source], banks, partial(turn, source, first))
+            for b in range(2):
+                step(("empty2", j, a, b), [banks[b]], [("w2in", j, q)], partial(empty, b))
+            quantize(("w2", j, q), E4M3, ("w2in", j, q))
 
-        def grad_job(j, g, behind=BEHIND, readers="ss"):
-            def fetch():
-                load(("grad", j, g), "small", [P, T, Y], BF16, grad_out[j].rearrange("(g p t) y -> g p t y", g=2, t=T)[g])
+        def grad(j, g):
+            load(("grad", j, g), "load", [P, T, Y], BF16, grad_out[j].rearrange("(g p t) y -> g p t y", g=2, t=T)[g])
+            specs["gin", j, g] = ("work", [P, K, T], BF16)
+            banks = banks_for(("gbank", j, g), 2, [P, 2, 2, P])
 
-            def turn():
+            def turn(engine):
                 words = tiles["grad", j, g][:].rearrange("p t y -> p (t y)").bitcast(F32).rearrange("p (t w) -> p t w", t=T)
                 for a in range(2):
-                    bank = take(("gbank", j, g, a), "bank", [P, 2, 2, P], F32)
                     for t in range(2):
                         for s in range(2):
-                            nc.tensor.transpose(bank[:, t, s, :], words[:, 2 * a + t, s::2], ident_f[:])
-                give(("grad", j, g))
+                            engine.transpose(tiles[banks[a]][:, t, s, :], words[:, 2 * a + t, s::2], ident_f[:])
 
-            def empty():
-                dst = take(("gin", j, g), "small", [P, K, T], BF16)[:].rearrange("p c t -> p (c t)").bitcast(F32)
-                for a in range(2):
-                    out = dst[:, cols(a, K)].rearrange("p (t m s) -> p t m s", t=2, s=2)
-                    copy(readers[a], out, tiles["gbank", j, g, a][:].rearrange("p t s m -> p t m s"))
-                    give(("gbank", j, g, a))
+            def empty(a, engine):
+                dst = tiles["gin", j, g][:].rearrange("p c t -> p (c t)").bitcast(F32)
+                out = dst[:, cols(a, K)].rearrange("p (t m s) -> p t m s", t=2, s=2)
+                copy(engine, out, tiles[banks[a]][:].rearrange("p t s m -> p t m s"))
 
-            quant = partial(quantize, ("g", j, g), E5M2, ("gin", j, g))
-            return [(-LOAD_LEAD - 1, DMA, fetch), (0, PE, turn), (1, READ, empty), (behind, QUANT, quant)]
+            step(("turng", j, g), [("grad", j, g)], banks, turn)
+            for a in range(2):
+                step(("emptyg", j, g, a), [banks[a]], [("gin", j, g)], partial(empty, a))
+            quantize(("g", j, g), E5M2, ("gin", j, g))
 
-        def x_steps(g, half, engines):
-            def fetch():
-                view = x.rearrange("(g p t) w -> g p t w", g=2, t=T)[g][:, :, cols(half, K)]
-                load(("x", g, half), "small", [P, T, K], BF16, view)
+        def x_part(g, xh):
+            load(("x", g, xh), "load", [P, T, K], BF16, x.rearrange("(g p t) w -> g p t w", g=2, t=T)[g][:, :, cols(xh, K)])
+            specs["xin", g, xh] = ("work", [P, K, T], BF16)
 
-            def interleave(n):
-                if n == 0:
-                    take(("xin", g, half), "small", [P, K, T], BF16, newest=engines[0] == "g")
-                src = tiles["x", g, half][:, :, cols(n, K // 2)].rearrange("p t (c i) -> p c t i", i=4)
-                copy(engines[n], tiles["xin", g, half][:, cols(n, K // 2), :].rearrange("p (c i) t -> p c t i", i=4), src)
-                if n == 1:
-                    give(("x", g, half))
+            def interleave(n, engine):
+                src = tiles["x", g, xh][:, :, cols(n, K // 2)].rearrange("p t (c i) -> p c t i", i=4)
+                copy(engine, tiles["xin", g, xh][:, cols(n, K // 2), :].rearrange("p (c i) t -> p c t i", i=4), src)
 
-            steps = [(0, POOL, partial(interleave, n)) if engines[n] == "g" else (n, MAKE, partial(interleave, n)) for n in range(2)]
-            quant = partial(quantize, ("xq", g, half), E4M3, ("xin", g, half))
-            return steps + [(-LOAD_LEAD, DMA, fetch), (BEHIND, QUANT, quant)]
+            for n in range(2):
+                step(("weave", g, xh, n), [("x", g, xh)], [("xin", g, xh)], partial(interleave, n))
+            quantize(("xq", g, xh), E4M3, ("xin", g, xh))
 
-        def w1_job(n, mean_first, pool_ahead=None, readers="ss"):
-            i, j = divmod(n, J)
+        def w1_pair(a):
+            for name, src in (("sig1", sig_W1), ("mu1", mu_W1)):
+                load((name, a), "load", [P, 2, H], BF16, src.rearrange("(a r m) h -> a m r h", r=2, m=P)[a])
+            specs["mean1", a] = ("work", [P, 2, T, 32, RUN], BF16)
+
+            def sort_mean(engine):
+                copy(engine, tiles["mean1", a][:], tiles["mu1", a][:].rearrange("p r (b u i) -> p r u b i", u=T, i=RUN))
+
+            step(("sort1", a), [("mu1", a)], [("mean1", a)], sort_mean)
+            for i in (2 * a, 2 * a + 1):
+                load(("e1", i), "load", [P, J, H], BF16, e_W1[:, cols(i), :].rearrange("j m h -> m j h"))
+                for j in range(J):
+                    w1_block(i, j)
+
+        def w1_block(i, j):
             a, r = divmod(i, 2)
             xh, c = divmod(i, 4)
-            sort = "p (b u i) -> p u b i"
+            n = J * i + j
+            specs["prod1", n] = ("work", [P, T, 32, RUN], F32)
+            specs["sum1", n] = ("work", [P, 2, 2 * P, 2], BF16)
+            specs["w1in", j, xh] = ("w1in", [P, 2 * K, T], BF16)
+            banks = banks_for(("w1bank", n), 2, [P, T, P])
+            specs["w1words", n] = ("bank", [P, 2, 2, P], F32)
 
-            def fetch():
-                if r == 0:
-                    load(("sig1", a), "small", [P, 2, H], BF16, sig_W1.rearrange("(a r m) h -> a m r h", r=2, m=P)[a])
-                load(("e1", i), "small", [P, J, H], BF16, e_W1[:, cols(i), :].rearrange("j m h -> m j h"))
-                if r == 0:
-                    load(("mu1", a), "small", [P, 2, H], BF16, mu_W1.rearrange("(a r m) h -> a m r h", r=2, m=P)[a])
-
-            def sort_mean():
-                dst = take(("mean1", a), "small", [P, 2, T, 32, RUN], BF16)
-                nc.vector.tensor_copy(out=dst[:], in_=tiles["mu1", a][:].rearrange("p r (b u i) -> p r u b i", u=T, i=RUN))
-                give(("mu1", a))
-
-            def multiply(engine, places):
-                if places.start == 0:
-                    take(("prod1", i, j), "small", [P, T, 32, RUN], F32, newest=pool_ahead is not None)
+            def multiply(engine):
+                sort = "p (b u i) -> p u b i"
                 engine.tensor_tensor(
-                    out=tiles["prod1", i, j][:, places],
-                    in0=tiles["e1", i][:, j, :].rearrange(sort, u=T, i=RUN)[:, places],
-                    in1=tiles["sig1", a][:, r, :].rearrange(sort, u=T, i=RUN)[:, places],
+                    out=tiles["prod1", n][:],
+                    in0=tiles["e1", i][:, j, :].rearrange(sort, u=T, i=RUN),
+                    in1=tiles["sig1", a][:, r, :].rearrange(sort, u=T, i=RUN),
                     op=ALU.mult,
                 )
-                if r == 1 and j == J - 1 and places.stop == T:
-                    give(("sig1", a))
 
-            def turn():
-                prod = tiles["prod1", i, j][:].rearrange("p u (q b) i -> p u q (b i)", q=2)
-                mean = tiles["mean1", a][:, r].rearrange("p u (q b) i -> p u q (b i)", q=2)
-                banks = [take(("w1bank", i, j, q), "bank", [P, T, P], F32) for q in range(2)]
-                transpose_sum(banks, lambda q, u: mean[:, u, q, :], lambda q, u: prod[:, u, q, :], mean_first)
-                give(("prod1", i, j))
-                if r == 1 and j == J - 1:
-                    give(("mean1", a))
+            def turn(is_mean, first, engine):
+                block = (tiles["mean1", a][:, r] if is_mean else tiles["prod1", n][:]).rearrange("p u (q b) i -> p u q (b i)", q=2)
+                turn_part(banks, lambda q, u: block[:, u, q, :], is_mean, first)
 
-            def empty():
+            def empty(q, engine):
+                copy(engine, tiles["w1in", j, xh][:, cols(T * q + c), :], tiles[banks[q]][:].rearrange("p u m -> p m u"))
+
+            def add_mean(engine):
+                pair = "p (s e) b i -> p s (b i) e"
+                engine.tensor_tensor(
+                    out=tiles["sum1", n][:],
+                    in0=tiles["prod1", n][:].rearrange(pair, e=2),
+                    in1=tiles["mean1", a][:, r].rearrange(pair, e=2),
+                    op=ALU.add,
+                )
+
+            def turn_words(engine):
+                words = tiles["sum1", n][:].rearrange("p s m e -> p (s m e)").bitcast(F32).rearrange("p (s q m) -> p q s m", s=2, q=2)
                 for q in range(2):
-                    if c == 0:
-                        take(("w1in", j, q, xh), "small", [P, K, T], BF16)
-                    src = tiles["w1bank", i, j, q][:].rearrange("p u m -> p m u")
-                    copy(readers[q], tiles["w1in", j, q, xh][:, cols(c), :], src)
-                    give(("w1bank", i, j, q))
+                    for s in range(2):
+                        engine.transpose(tiles["w1words", n][:, q, s, :], words[:, q, s, :], ident_f[:])
 
-            steps = [(0, PE, turn), (1, READ, empty)]
-            if pool_ahead is None:
-                steps.append((-W1_AHEAD, MAKE, partial(multiply, nc.vector, slice(0, T))))
-            else:
-                steps.append((-pool_ahead, POOL, partial(multiply, nc.gpsimd, slice(0, POOL_PLACES))))
-                steps.append((-pool_ahead + 1, MAKE, partial(multiply, nc.vector, slice(POOL_PLACES, T))))
-            if j == 0:
-                steps.append((-LOAD_LEAD - W2_AHEAD, DMA, fetch))
-                if r == 0:
-                    steps.append((-W1_AHEAD, MAKE, sort_mean))
-            if c == 3:
-                for q in range(2):
-                    steps.append((BEHIND + q, QUANT, partial(quantize, ("w1", j, q, xh), E4M3, ("w1in", j, q, xh))))
-            return steps
+            def empty_words(engine):
+                dst = tiles["w1in", j, xh][:].rearrange("p c t -> p (c t)").bitcast(F32).rearrange("p (q c m s) -> p q c m s", q=2, m=P, s=2)
+                copy(engine, dst[:, :, c], tiles["w1words", n][:].rearrange("p q s m -> p q m s"))
 
-        def dh_jobs(key, abs_ahead, quant_behind):
-            j, q, g = key
+            step(("mul1", n), [("e1", i), ("sig1", a)], [("prod1", n)], multiply)
+            for first in (False, True):
+                step(("turn1", n, first), [("prod1", n)], banks, partial(turn, False, first))
+                step(("mean1", n, first), [("mean1", a)], banks, partial(turn, True, first))
+            for q in range(2):
+                step(("empty1", n, q), [banks[q]], [("w1in", j, xh)], partial(empty, q))
+            step(("add1", n), [("prod1", n), ("mean1", a)], [("sum1", n)], add_mean)
+            step(("turn1w", n), [("sum1", n)], [("w1words", n)], turn_words)
+            step(("empty1w", n), [("w1words", n)], [("w1in", j, xh)], empty_words)
+            quantize(("w1", j, xh), E4M3, ("w1in", j, xh), kind="wide")
 
-            def fetch():
-                view = z1[j].rearrange("(g p t) h -> g p t h", g=2, t=T)[g][:, :, cols(q, K)]
-                load(("z",) + key, "large", [P, T, K], F32, view)
+        def unit(k):
+            j, q, g = UNITS[k]
+            load(("z", k), "z", [P, T, K], F32, z1[j].rearrange("(g p t) h -> g p t h", g=2, t=T)[g][:, :, cols(q, K)])
+            for name in ("abs", "dz", "dzin"):
+                specs[name, k] = ("work", [P, K, T], BF16)
+            dh = banks_for(("dhbank", k), T, [P, T, P])
+            turned = banks_for(("dzbank", k), 2, [P, T, P])
 
-            def absolute(n):
-                if n == 0:
-                    take(("abs",) + key, "small", [P, K, T], BF16)
-                dst = tiles[("abs",) + key][:, cols(n, K // 2), :].rearrange("p (c i) t -> p c t i", i=4)
-                src = tiles[("z",) + key][:, :, cols(n, K // 2)].rearrange("p t (c i) -> p c t i", i=4)
-                nc.scalar.activation(out=dst, in_=src, func=ACT.Abs, scale=EDGE)
-                if n == 1:
-                    give(("z",) + key)
+            def absolute(n, engine):
+                dst = tiles["abs", k][:, cols(n, K // 2), :].rearrange("p (c i) t -> p c t i", i=4)
+                src = tiles["z", k][:, :, cols(n, K // 2)].rearrange("p t (c i) -> p c t i", i=4)
+                engine.activation(out=dst, in_=src, func=ACT.Abs, scale=EDGE)
 
-            def multiply(half):
-                for u in (2 * half, 2 * half + 1):
-                    bank = take(("dh",) + key + (u,), "bank", [P, T, P], F32)
-                    for t in range(T):
-                        mx(bank[:, t, :], ("g", j, g), cols(t), E5M2, ("w2", j, q), cols(u), E4M3, True, True)
-                if half == 1 and q == 1:
-                    give(("g", j, g))
-                if half == 1 and g == 1:
-                    give(("w2", j, q))
+            def multiply(u, engine):
+                for t in range(T):
+                    mx(tiles[dh[u]][:, t, :], ("g", j, g), cols(t), E5M2, ("w2", j, q), cols(u), E4M3, True, True)
 
-            def mask():
-                dz = take(("dz",) + key, "small", [P, K, T], BF16)[:].rearrange("p (u b i) t -> p u b i t", u=T, i=RUN)
-                size = tiles[("abs",) + key][:].rearrange("p (b u i) t -> p u b i t", u=T, i=RUN)
+            def mask(u, engine):
+                dz = tiles["dz", k][:].rearrange("p (u b i) t -> p u b i t", u=T, i=RUN)
+                size = tiles["abs", k][:].rearrange("p (b u i) t -> p u b i t", u=T, i=RUN)
+                bank = tiles[dh[u]][:].rearrange("p t (b i) -> p b i t", i=RUN)
+                engine.scalar_tensor_tensor(out=dz[:, u], in0=size[:, u], scalar=EDGE, in1=bank, op0=ALU.is_lt, op1=ALU.mult)
+
+            def turn(s, engine):
+                words = tiles["dz", k][:].rearrange("p c t -> p (c t)").bitcast(F32).rearrange("p (u m s) -> p s u m", u=T, s=2)
                 for u in range(T):
-                    bank = tiles[("dh",) + key + (u,)][:].rearrange("p t (b i) -> p b i t", i=RUN)
-                    nc.vector.scalar_tensor_tensor(out=dz[:, u], in0=size[:, u], scalar=EDGE, in1=bank, op0=ALU.is_lt, op1=ALU.mult)
-                    give(("dh",) + key + (u,))
-                give(("abs",) + key)
+                    engine.transpose(tiles[turned[s]][:, u, :], words[:, s, u, :], ident_f[:])
 
-            quant = partial(quantize, ("dzn",) + key, E5M2, ("dz",) + key, last_reader=False)
-            first = [(0, PE, partial(multiply, 0)), (-LOAD_LEAD - abs_ahead - 1, DMA, fetch)]
-            first += [(n - abs_ahead, MAKE, partial(absolute, n)) for n in range(2)]
-            second = [(0, PE, partial(multiply, 1)), (1, READ, mask), (quant_behind, QUANT, quant)]
-            return first, second
+            def empty(s, engine):
+                src = tiles[turned[s]][:].bitcast(BF16).rearrange("p u (m e) -> p e m u", e=2)
+                copy(engine, tiles["dzin", k][:, cols(s, K // 2), :].rearrange("p (e m) u -> p e m u", e=2), src)
 
-        def dz_job(key, behind):
-            def turn():
-                words = tiles[("dz",) + key][:].rearrange("p c t -> p (c t)").bitcast(F32).rearrange("p (u m s) -> p s u m", u=T, s=2)
-                for s in range(2):
-                    bank = take(("dzbank",) + key + (s,), "bank", [P, T, P], F32)
-                    for u in range(T):
-                        nc.tensor.transpose(bank[:, u, :], words[:, s, u, :], ident_f[:])
-                give(("dz",) + key)
+            for n in range(2):
+                step(("abs", k, n), [("z", k)], [("abs", k)], partial(absolute, n))
+                step(("turnz", k, n), [("dz", k)], [turned[n]], partial(turn, n))
+                step(("emptyz", k, n), [turned[n]], [("dzin", k)], partial(empty, n))
+            for u in range(T):
+                step(("dh", k, u), [("g", j, g), ("w2", j, q)], [dh[u]], partial(multiply, u))
+                step(("mask", k, u), [("abs", k), dh[u]], [("dz", k)], partial(mask, u))
+            quantize(("dzn", j, q, g), E5M2, ("dz", k))
+            quantize(("dzh", j, q, g), E5M2, ("dzin", k))
 
-            def empty():
-                dst = take(("dzin",) + key, "small", [P, K, T], BF16)
-                for s in range(2):
-                    src = tiles[("dzbank",) + key + (s,)][:].bitcast(BF16).rearrange("p u (m e) -> p e m u", e=2)
-                    nc.scalar.copy(out=dst[:, cols(s, K // 2), :].rearrange("p (e m) u -> p e m u", e=2), in_=src)
-                    give(("dzbank",) + key + (s,))
+        def dx(g, xh, t):
+            bank = ("dxbank", g, xh, t)
+            specs[bank] = ("bank", [P, K], F32)
+            specs["out0", g, xh, t] = ("work", [P, K], F32)
+            passes = [(q, j) for q in range(2) for j in range(J)]
 
-            quant = partial(quantize, ("dzh",) + key, E5M2, ("dzin",) + key)
-            return [(0, PE, turn), (1, READ, empty), (behind, QUANT, quant)]
+            def multiply(engine):
+                for q, j in passes:
+                    mx(tiles[bank][:], ("dzh", j, q, g), cols(t), E5M2, ("w1", j, xh), cols(q, K), E4M3, (q, j) == passes[0], (q, j) == passes[-1])
 
-        def dx_job(g, xh, t, together=1, piece=0, pieces=1, reader="s"):
-            width = K // pieces
-            bank_key = ("dx", g, xh, t, piece)
-            out_key = ("out0", g, xh, t // together, piece)
-
-            def multiply():
-                bank = take(bank_key, "bank", [P, width], F32)
-                for k in range(2 * J):
-                    q, j = divmod(k, J)
-                    mx(bank[:], ("dzh", j, q, g), cols(t), E5M2, ("w1", j, q, xh), cols(piece, width), E4M3, k == 0, k == 2 * J - 1)
-                    if t == T - 1 and xh == 1 and g == 0:
-                        give(("dzh", j, q, g))
-                    if t == T - 1 and xh == 0 and g == 1:
-                        give(("w1", j, q, xh))
-
-            def empty():
-                if t % together == 0:
-                    take(out_key, "small", [P, together, width], F32)
-                copy(reader, tiles[out_key][:, t % together, :], tiles[bank_key][:])
-                give(bank_key)
-
-            def store():
+            def store(engine):
                 view = out_0.rearrange("(g p t) w -> g p t w", g=2, t=T)[g]
-                nc.sync.dma_start(out=view[:, cols(t // together, together), cols(pieces * xh + piece, width)], in_=tiles[out_key][:])
-                give(out_key)
+                engine.dma_start(out=view[:, t, cols(xh, K)], in_=tiles["out0", g, xh, t][:])
 
-            steps = [(0, PE, multiply), (1, READ, empty)]
-            return steps + ([(1, DMA, store)] if t % together == together - 1 else [])
+            step(("dx", g, xh, t), [("dzh", j, q, g) for q, j in passes] + [("w1", j, xh) for j in range(J)], [bank], multiply)
+            step(("emptyx", g, xh, t), [bank], [("out0", g, xh, t)], lambda engine: copy(engine, tiles["out0", g, xh, t][:], tiles[bank][:]))
+            step(("store0", g, xh, t), [("out0", g, xh, t)], [], store)
 
-        def dw_job(q, items, adders, store_behind):
+        def dw(q, i, j):
+            bank = ("dwbank", q, i, j)
+            part = ("part", q, i // 2, j)
+            specs[bank] = ("bank", [P, K], F32)
+            specs[part] = ("work", [P, 2, K], F32)
             natural = "p (b u i) -> p b u i"
 
-            def multiply():
-                for i, j in items:
-                    bank = take(("dw", q, i, j), "bank", [P, K], F32)
-                    for g in range(2):
-                        mx(bank[:], ("xq", g, i // 4), cols(i % 4), E4M3, ("dzn", j, q, g), cols(0, K), E5M2, g == 0, g == 1)
-                        if i == X // P - 1:
-                            give(("dzn", j, q, g))
+            def multiply(engine):
+                for g in range(2):
+                    mx(tiles[bank][:], ("xq", g, i // 4), cols(i % 4), E4M3, ("dzn", j, q, g), cols(0, K), E5M2, g == 0, g == 1)
 
-            def weigh():
-                for i, j in items:
-                    if i % 2 == 0:
-                        take(("part", q, i // 2, j), "small", [P, 2, K], F32)
-                    nc.vector.tensor_tensor(
-                        out=tiles["part", q, i // 2, j][:, i % 2, :].rearrange(natural, u=T, i=RUN),
-                        in0=tiles["e1", i][:, j, cols(q, K)].rearrange(natural, u=T, i=RUN),
-                        in1=tiles["dw", q, i, j][:].rearrange("p (u b i) -> p b u i", u=T, i=RUN),
-                        op=ALU.mult,
-                    )
-                    give(("dw", q, i, j))
-                    if q == 1 and j == J - 1:
-                        give(("e1", i))
+            def weigh(engine):
+                engine.tensor_tensor(
+                    out=tiles[part][:, i % 2, :].rearrange(natural, u=T, i=RUN),
+                    in0=tiles["e1", i][:, j, cols(q, K)].rearrange(natural, u=T, i=RUN),
+                    in1=tiles[bank][:].rearrange("p (u b i) -> p b u i", u=T, i=RUN),
+                    op=ALU.mult,
+                )
 
-            def add(i):
-                total = tiles["part", q, i // 2, 0][:, i % 2, :]
-                engine = nc.gpsimd if adders[i] == "g" else nc.vector
-                engine.tensor_tensor(out=total, in0=total, in1=tiles["part", q, i // 2, 1][:, i % 2, :], op=ALU.add)
-                if i % 2 == 1:
-                    give(("part", q, i // 2, 1))
+            step(("dw", q, i, j), [("xq", g, i // 4) for g in range(2)] + [("dzn", j, q, g) for g in range(2)], [bank], multiply)
+            step(("weigh", q, i, j), [("e1", i), bank], [part], weigh)
 
-            def store(i):
-                view = out_1.rearrange("(a r m) h -> a m r h", r=2, m=P)[i // 2][:, :, cols(q, K)]
-                nc.sync.dma_start(out=view, in_=tiles["part", q, i // 2, 0][:])
-                give(("part", q, i // 2, 0))
+        def dw_sum(q, a):
+            first, second, total = ("part", q, a, 0), ("part", q, a, 1), ("total", q, a)
+            specs[total] = ("work", [P, 2, K], F32)
 
-            done = [i for i, j in items if j == J - 1]
-            steps = [(0, PE, multiply), (1, READ, weigh)] + [(1, MAKE, partial(add, i)) for i in done]
-            return steps + [(store_behind, DMA, partial(store, i)) for i in done if i % 2 == 1]
+            def add(engine):
+                engine.tensor_tensor(out=tiles[total][:], in0=tiles[first][:], in1=tiles[second][:], op=ALU.add)
 
-        jobs = []
-        starts = []
+            def store(engine):
+                view = out_1.rearrange("(a r m) h -> a m r h", r=2, m=P)[a][:, :, cols(q, K)]
+                engine.dma_start(out=view, in_=tiles[total][:])
 
-        def unit(key, early, late, beside=(), quant_behind=2, last=False):
-            abs_ahead = len(jobs) - starts[-1] - 2 if len(starts) > 1 else 2 + len(starts)
-            starts.append(len(jobs))
-            first, second = dh_jobs(key, abs_ahead, quant_behind)
-            jobs.extend([first, second + list(beside)] + early + [dz_job(key, 2 if last else len(late) + 2)] + late)
+            step(("sum", q, a), [first, second], [total], add)
+            step(("store1", q, a), [total], [], store)
 
-        def weave(first, second):
-            woven = []
-            for n in range(max(len(first), len(second))):
-                woven += first[n : n + 1] + second[n : n + 1]
-            return woven
+        for a in range(4):
+            w2_rows(a)
+            w1_pair(a)
+            grad(*divmod(a, 2))
+            x_part(*divmod(a, 2))
+            for q in range(2):
+                dw_sum(q, a)
+        for k in range(len(UNITS)):
+            unit(k)
+            for half in range(2):
+                dx(half, *divmod(k, T))
+                for j in range(J):
+                    dw(half, k, j)
 
-        jobs.extend([w2_job(0, 0, 0, False), w2_job(0, 0, 1, True, behind=2), grad_job(0, 0, behind=1, readers="vv"), w2_job(1, 0, 0, False)])
-        unit(
-            (0, 0, 0),
-            [w2_job(1, 0, 1, True), grad_job(1, 0)],
-            [w2_job(0, 1, 0, False), w2_job(0, 1, 1, True), w2_job(1, 1, 0, False)],
-        )
-        unit((1, 0, 0), [w2_job(1, 1, 1, True), w1_job(0, False), w1_job(1, True, pool_ahead=3)], [w1_job(2, False)])
-        unit(
-            (0, 1, 0),
-            [w1_job(3, True), w1_job(4, False), w1_job(5, True, pool_ahead=3, readers="vs")],
-            [w1_job(6, False), w1_job(7, False)],
-        )
-        unit(
-            (1, 1, 0),
-            [w1_job(8, True), grad_job(0, 1, behind=BEHIND + 1), w1_job(9, True)],
-            [w1_job(10, False) + x_steps(0, 1, "vv"), w1_job(11, True), grad_job(1, 1, behind=BEHIND + 1)],
-            beside=x_steps(0, 0, "gv"),
-        )
-        dx = [dx_job(0, 0, t, together=2) for t in range(T)]
-        unit(
-            (0, 0, 1),
-            [dx[0], dx[1], w1_job(12, True)],
-            [w1_job(13, False), dx[2] + x_steps(1, 1, "vv"), dx[3]],
-            beside=x_steps(1, 0, "gv"),
-        )
-        rows = X // P
-        dw = [dw_job(0, [(i, 0), (i + 1, 0)], "", 1) for i in range(0, rows, 2)]
-        unit(
-            (1, 0, 1),
-            [dw[0], dw[1], w1_job(14, True, pool_ahead=3)],
-            [w1_job(15, False, pool_ahead=3), dw[2], dw[3]],
-            quant_behind=3,
-        )
-        dx = [dx_job(0, 1, t, together=2) for t in range(T)]
-        dw = [dw_job(0, [(i, 1), (i + 1, 1)], "g" * rows, 1) for i in range(0, rows, 2)]
-        unit((0, 1, 1), dw[:2] + dx[:1], weave(dw[2:], dx[1:]))
-        items = [(i, j) for j in range(J) for i in range(rows // 2)] + [(i, j) for i in range(rows // 2, rows) for j in range(J)]
-        dw = [dw_job(1, items[n : n + 2], "vgvg" + "gggg", BEHIND) for n in range(0, len(items), 2)]
-        unit((1, 1, 1), dw[:2], dw[2:6], last=True)
-        dx = [dx_job(1, xh, t) for xh in range(2) for t in range(T)][:-1]
-        dx += [dx_job(1, 1, T - 1, piece=n, pieces=2, reader="sv"[n]) for n in range(2)]
-        jobs.extend(weave(dx, dw[6:]))
+        pe, dve, act, pool, sp = [], [], [], [], []
+        inherits = {}
 
-        steps = []
-        for place in range(len(jobs)):
-            for offset, rank, step in jobs[place]:
-                steps.append((place + offset, rank, len(steps), step))
-        for at, rank, n, step in sorted(steps):
-            step()
+
+        def two(*name):
+            return [name + (0,), name + (1,)]
+
+        def four(*name):
+            return [name + (n,) for n in range(T)]
+
+        def loads(*keys):
+            return [("load",) + key for key in keys]
+
+        def quant(*key):
+            return [("quant",) + key]
+
+        def dzn(k):
+            return quant("dzn", *UNITS[k])
+
+        def dzh(k):
+            return quant("dzh", *UNITS[k])
+
+        def on_pool(name, tile, after):
+            pool.append(name)
+            inherits[tile] = after
+
+        def dws(kind, q, j, rows):
+            return [(kind, q, i, j) for i in rows]
+
+        def open_with(name, *key):
+            return [(name,) + key + (True,)]
+
+        def close_with(name, *key):
+            return [(name,) + key + (False,)]
+
+        def w2(j, a, mean):
+            return (("turn2", j, a), (mean, j, a))
+
+        def w1(n):
+            return (("turn1", n), ("mean1", n))
+
+        def products_first(*jobs):
+            return [job[0] + (True,) for job in jobs] + [job[1] + (False,) for job in jobs]
+
+        def means_first(*jobs):
+            return [job[1] + (True,) for job in jobs] + [job[0] + (False,) for job in jobs]
+
+        def around(a, b):
+            return means_first(a) + products_first(b)
+
+        sp += loads(("sig2", 0), ("e2", 0, 0), ("mu2", 0), ("sig2", 1), ("e2", 0, 1), ("mu2", 1), ("grad", 0, 0), ("e2", 1, 0), ("e2", 1, 1), ("z", 0))
+        sp += loads(("grad", 1, 0), ("sig2", 2), ("e2", 0, 2), ("mu2", 2), ("z", 1), ("sig2", 3), ("e2", 0, 3), ("mu2", 3), ("e2", 1, 2), ("e2", 1, 3))
+        sp += loads(("sig1", 0), ("e1", 0), ("mu1", 0), ("z", 2), ("e1", 1), ("sig1", 1), ("e1", 2), ("mu1", 1), ("z", 3), ("grad", 0, 1), ("e1", 3))
+        sp += loads(("x", 0, 0), ("z", 4), ("grad", 1, 1), ("x", 1, 0), ("sig1", 2), ("e1", 4), ("mu1", 2), ("x", 0, 1), ("z", 5), ("x", 1, 1), ("e1", 5))
+        sp += loads(("e1", 6), ("sig1", 3), ("mu1", 3), ("z", 6), ("e1", 7))
+        sp += four("store0", 0, 0) + loads(("z", 7))
+        pe += products_first(w2(0, 0, "mean2")) + means_first(w2(0, 1, "mean2")) + [("turng", 0, 0)] + around(w2(1, 0, "mean2"), w2(1, 1, "mean2"))
+        dve += [("mul2", 0, 0), ("mul2", 0, 1), ("mul2", 1, 0), ("mul2", 1, 1)] + two("emptyg", 0, 0) + quant("w2", 0, 0) + quant("g", 0, 0) + [("empty2", 1, 0, 0)]
+        act += [("sort2", 0), ("sort2", 1)] + two("empty2", 0, 0) + two("empty2", 0, 1) + two("abs", 0) + [("empty2", 1, 0, 1)] + two("empty2", 1, 1)
+        pe += four("dh", 0) + [("turng", 1, 0)] + open_with("raw2", 0, 2) + two("turnz", 0) + open_with("raw2", 0, 3) + close_with("turn2", 0, 2) + close_with("turn2", 0, 3)
+        dve += four("mask", 0) + [("mul2", 0, 2)] + dzn(0) + [("mul2", 0, 3)] + quant("w2", 1, 0) + [("mul2", 1, 2)] + quant("g", 1, 0) + [("mul2", 1, 3)] + dzh(0)
+        act += two("emptyg", 1, 0) + [("abs", 1, 0)] + two("emptyz", 0) + [("abs", 1, 1)] + two("empty2", 0, 2) + two("empty2", 0, 3)
+        pe += four("dh", 1) + products_first(w2(1, 2, "raw2"), w2(1, 3, "raw2")) + two("turnz", 1) + around(w1(0), w1(1))
+        dve += four("mask", 1) + [("sort1", 0)] + dzn(1) + [("mul1", 1)] + quant("w2", 0, 1) + [("mul1", 2), ("mul1", 3)] + quant("w2", 1, 1) + [("sort1", 1)] + dzh(1)
+        on_pool(("mul1", 0), ("prod1", 0), ("dzin", 0))
+        act += two("abs", 2) + two("empty2", 1, 2) + two("empty2", 1, 3) + two("emptyz", 1) + two("empty1", 0) + two("empty1", 1)
+        pe += four("dh", 2) + products_first(w1(2), w1(3)) + two("turnz", 2) + open_with("mean1", 4) + [("turng", 0, 1)] + open_with("mean1", 5) + close_with("turn1", 4) + close_with("turn1", 5)
+        dve += four("mask", 2) + two("empty1", 2) + [("mul1", 5)] + dzn(2) + [("mul1", 6)] + two("emptyg", 0, 1) + [("mul1", 7)] + dzh(2)
+        on_pool(("mul1", 4), ("prod1", 4), ("dzin", 1))
+        act += two("abs", 3) + two("empty1", 3) + two("emptyz", 2) + two("empty1", 4) + two("empty1", 5)
+        pe += four("dh", 3) + around(w1(6), w1(7)) + two("turnz", 3) + open_with("mean1", 8) + [("turng", 1, 1)] + close_with("turn1", 8)
+        dve += four("mask", 3) + [("empty1", 6, 1), ("sort1", 2)] + dzn(3) + quant("g", 0, 1) + quant("w1", 0, 0) + two("weave", 0, 0) + quant("w1", 1, 0) + dzh(3)
+        on_pool(("mul1", 8), ("prod1", 8), ("dzin", 2))
+        act += two("abs", 4) + [("empty1", 6, 0)] + two("empty1", 7) + two("emptyz", 3) + two("emptyg", 1, 1)
+        pe += four("dh", 4) + [("dx", 0, 0, 0), ("dx", 0, 0, 1)] + two("turnz", 4) + [("dx", 0, 0, 2)] + means_first(w1(9)) + [("dx", 0, 0, 3)]
+        dve += four("mask", 4) + quant("xq", 0, 0) + dzn(4) + quant("g", 1, 1) + two("weave", 1, 0) + two("weave", 0, 1) + quant("xq", 1, 0) + quant("xq", 0, 1) + dzh(4)
+        on_pool(("mul1", 9), ("prod1", 9), ("dzin", 3))
+        act += two("empty1", 8) + two("abs", 5) + [("emptyx", 0, 0, 0), ("emptyx", 0, 0, 1)] + two("emptyz", 4) + [("emptyx", 0, 0, 2)] + two("empty1", 9) + [("emptyx", 0, 0, 3)]
+        pe += four("dh", 5) + dws("dw", 0, 0, range(4)) + two("turnz", 5) + around(w1(10), w1(11)) + dws("dw", 0, 0, range(4, 8))
+        dve += four("mask", 5) + dws("weigh", 0, 0, range(4)) + dzn(5) + quant("xq", 1, 1) + [("sort1", 3), ("mul1", 12)] + dzh(5) + dws("weigh", 0, 0, range(4, 8))
+        on_pool(("mul1", 10), ("prod1", 10), ("dzin", 4))
+        pool.append(("mul1", 11))
+        act += two("weave", 1, 1) + two("emptyz", 5) + two("abs", 6) + two("empty1", 10) + two("empty1", 11)
+        pe += four("dh", 6) + around(w1(12), w1(13)) + two("turnz", 6) + dws("dw", 0, 1, range(8))
+        dve += four("mask", 6) + [("mul1", 15)] + dzn(6) + dws("weigh", 0, 1, range(8))
+        on_pool(("mul1", 13), ("prod1", 13), ("dzin", 5))
+        pool += [("mul1", 14)]
+        act += two("abs", 7) + two("empty1", 12) + two("empty1", 13) + two("emptyz", 6)
+        pe += four("dh", 7) + dws("dw", 1, 0, range(4)) + two("turnz", 7) + dws("dw", 1, 0, range(4, 8))
+        dve += four("mask", 7) + dws("weigh", 1, 0, range(4)) + dzn(7) + dzh(6) + dzh(7) + dws("weigh", 1, 0, range(4, 8))
+        pool += four("sum", 0)[:3]
+        on_pool(("sum", 0, 3), ("total", 0, 3), ("dzin", 7))
+        act += two("emptyz", 7)
+        sp += four("store1", 0)[:3]
+        pe += four("dx", 1, 0)[:3] + [("turn1w", 14), ("turn1w", 15), ("dx", 1, 0, 3)] + dws("dw", 1, 1, range(8))
+        pe += four("dx", 0, 1) + four("dx", 1, 1)
+        dve += [("add1", 14), ("add1", 15)] + quant("w1", 0, 1) + quant("w1", 1, 1) + dws("weigh", 1, 1, range(8)) + four("sum", 1)[1:]
+        pool.append(("sum", 1, 0))
+        act += four("emptyx", 1, 0)[:3] + [("empty1w", 14), ("empty1w", 15), ("emptyx", 1, 0, 3)] + four("emptyx", 0, 1) + four("emptyx", 1, 1)
+        sp += [("store0", 1, 0, 0), ("store1", 0, 3)] + four("store0", 1, 0)[1:]
+        for n in range(T):
+            sp += [("store1", 1, n), ("store0", 0, 1, n)]
+        sp += four("store0", 1, 1)
+
+
+        queues = [(nc.tensor, pe), (nc.vector, dve), (nc.scalar, act), (nc.gpsimd, pool), (nc.sync, sp)]
+        writers = {}
+        readers = {}
+        for engine, queue in queues:
+            for name in queue:
+                for key in steps[name][0]:
+                    readers[key] = readers.get(key, 0) + 1
+                for key in steps[name][1]:
+                    writers[key] = writers.get(key, 0) + 1
+        heirs = {old: new for new, old in inherits.items()}
+        free = {kind: list(range(count)) for kind, count in SLOTS.items()}
+        slots = {}
+
+        def fresh(name):
+            return [key for key in steps[name][1] if key in specs and key not in tiles]
+
+        def ready(name):
+            kinds = [specs[key][0] for key in fresh(name) if key not in inherits]
+            return (
+                all(writers[key] == 0 for key in steps[name][0])
+                and all(len(free[kind]) >= sum(other == kind for other in kinds) for kind in kinds)
+                and all(key in slots for key in fresh(name) if key in inherits)
+            )
+
+        def take(key):
+            kind, shape, dtype = specs[key]
+            if key not in inherits:
+                slots[key] = free[kind].pop(0)
+            tag = "%s%d" % (kind, slots[key])
+            if kind == "bank":
+                tiles[key] = psum.tile(shape, dtype, name=key[0], tag=tag)
+            elif kind in ("code", "wide"):
+                words = sbuf.tile(shape, U32, name=key[0], tag=tag, align_bytes=64)
+                scales = sbuf.tile(shape, U8, name=key[0] + "_s", tag=tag + "_s", align_bytes=64)
+                tiles[key] = (words, scales)
+            else:
+                tiles[key] = sbuf.tile(shape, dtype, name=key[0], tag=tag, align_bytes=64)
+
+        def emit(engine, name):
+            reads, writes, work = steps[name]
+            for key in fresh(name):
+                take(key)
+            work(engine)
+            for key in writes:
+                writers[key] -= 1
+            for key in reads:
+                readers[key] -= 1
+                if readers[key] == 0 and key in heirs:
+                    slots[heirs[key]] = slots[key]
+                elif readers[key] == 0 and key in specs:
+                    free[specs[key][0]].append(slots[key])
+
+        while any(queue for engine, queue in queues):
+            heads = [(engine, queue) for engine, queue in queues if queue and ready(queue[0])]
+            assert heads, [queue[:1] for engine, queue in queues]
+            for engine, queue in heads:
+                if ready(queue[0]):
+                    emit(engine, queue.pop(0))

@@ -27,7 +27,7 @@ EDGE = 1.0 + 3.0 / 256.0
 
 UNITS = [(j, q, g) for g in range(2) for q in range(2) for j in range(J)]
 
-SLOTS = {"load": 14, "work": 16, "z": 3, "w1in": 2, "code": 22, "wide": 4, "bank": 8}
+SLOTS = {"load": 13, "work": 17, "z": 3, "w1in": 2, "code": 22, "wide": 4, "bank": 8}
 
 
 def tile_gaussian_nn_htanh_v_kernel(
@@ -103,22 +103,29 @@ def tile_gaussian_nn_htanh_v_kernel(
                 specs[name] = ("bank", shape, F32)
             return names
 
+        def w2_load(src, name, a):
+            blocks = 2 if a < 2 else 4
+            load(name + (min(a, 2),), "load", [P, blocks, Y], BF16, src.rearrange("(a b m) y -> a m b y", b=blocks, m=P)[a if a < 2 else 1])
+
+        def w2_in(name, a):
+            return tiles[name + (min(a, 2),)][:, cols(max(a - 2, 0), 2), :]
+
         def w2_rows(a):
             q, r = divmod(a, 2)
             for name, src in (("sig2", sig_W2), ("mu2", mu_W2)):
-                load((name, a), "load", [P, 2, Y], BF16, src.rearrange("(a b m) y -> a m b y", b=2, m=P)[a])
+                w2_load(src, (name,), a)
             specs["mean2", a] = ("work", [P, T, 2, P], BF16)
 
             def sort_mean(engine):
-                src = tiles["mu2", a][:].rearrange("p b (w i t) -> p (b w) t i", t=T, i=4)
+                src = w2_in(("mu2",), a).rearrange("p b (w i t) -> p (b w) t i", t=T, i=4)
                 copy(engine, tiles["mean2", a][:].rearrange("p t b (w i) -> p (b w) t i", i=4), src)
 
-            step(("sort2", a), [("mu2", a)], [("mean2", a)], sort_mean)
+            step(("sort2", a), [("mu2", min(a, 2))], [("mean2", a)], sort_mean)
             for j in range(J):
                 w2_sample(j, a, q, r)
 
         def w2_sample(j, a, q, r):
-            load(("e2", j, a), "load", [P, 2, Y], BF16, e_W2[j].rearrange("(a b m) y -> a m b y", b=2, m=P)[a])
+            w2_load(e_W2[j], ("e2", j), a)
             specs["prod2", j, a] = ("work", [P, T, 2, P], F32)
             specs["w2in", j, q] = ("work", [P, K, T], BF16)
             banks = banks_for(("w2bank", j, a), 2, [P, T, P])
@@ -127,13 +134,13 @@ def tile_gaussian_nn_htanh_v_kernel(
                 walk = "p b (w i t) -> p (b w) t i"
                 engine.tensor_tensor(
                     out=tiles["prod2", j, a][:].rearrange("p t b (w i) -> p (b w) t i", i=2),
-                    in0=tiles["e2", j, a][:].rearrange(walk, t=T, i=2),
-                    in1=tiles["sig2", a][:].rearrange(walk, t=T, i=2),
+                    in0=w2_in(("e2", j), a).rearrange(walk, t=T, i=2),
+                    in1=w2_in(("sig2",), a).rearrange(walk, t=T, i=2),
                     op=ALU.mult,
                 )
 
             def turn(source, first, engine):
-                block = tiles[source][:].rearrange("p b (w t) -> p t b w", t=T) if source[0] == "mu2" else tiles[source]
+                block = w2_in(("mu2",), a).rearrange("p b (w t) -> p t b w", t=T) if source[0] == "mu2" else tiles[source]
                 turn_part(banks, lambda b, t: block[:, t, b, :], source[0] != "prod2", first)
 
             def empty(b, engine):
@@ -141,9 +148,9 @@ def tile_gaussian_nn_htanh_v_kernel(
                 src = tiles[banks[b]][:].rearrange("p t (b u i) -> p u b i t", u=T, i=RUN)
                 copy(engine, dst[:, :, cols(2 * r + b, 4), :, :], src)
 
-            step(("mul2", j, a), [("e2", j, a), ("sig2", a)], [("prod2", j, a)], multiply)
+            step(("mul2", j, a), [("e2", j, min(a, 2)), ("sig2", min(a, 2))], [("prod2", j, a)], multiply)
             for first in (False, True):
-                for name, source in (("turn2", ("prod2", j, a)), ("mean2", ("mean2", a)), ("raw2", ("mu2", a))):
+                for name, source in (("turn2", ("prod2", j, a)), ("mean2", ("mean2", a)), ("raw2", ("mu2", min(a, 2)))):
                     step((name, j, a, first), [source], banks, partial(turn, source, first))
             for b in range(2):
                 step(("empty2", j, a, b), [banks[b]], [("w2in", j, q)], partial(empty, b))
@@ -207,12 +214,12 @@ def tile_gaussian_nn_htanh_v_kernel(
             banks = banks_for(("w1bank", n), 2, [P, T, P])
             specs["w1words", n] = ("bank", [P, 2, 2, P], F32)
 
-            def multiply(engine):
+            def multiply(places, engine):
                 sort = "p (b u i) -> p u b i"
                 engine.tensor_tensor(
-                    out=tiles["prod1", n][:],
-                    in0=tiles["e1", i][:, j, :].rearrange(sort, u=T, i=RUN),
-                    in1=tiles["sig1", a][:, r, :].rearrange(sort, u=T, i=RUN),
+                    out=tiles["prod1", n][:, places],
+                    in0=tiles["e1", i][:, j, :].rearrange(sort, u=T, i=RUN)[:, places],
+                    in1=tiles["sig1", a][:, r, :].rearrange(sort, u=T, i=RUN)[:, places],
                     op=ALU.mult,
                 )
 
@@ -242,7 +249,8 @@ def tile_gaussian_nn_htanh_v_kernel(
                 dst = tiles["w1in", j, xh][:].rearrange("p c t -> p (c t)").bitcast(F32).rearrange("p (q c m s) -> p q c m s", q=2, m=P, s=2)
                 copy(engine, dst[:, :, c], tiles["w1words", n][:].rearrange("p q s m -> p q m s"))
 
-            step(("mul1", n), [("e1", i), ("sig1", a)], [("prod1", n)], multiply)
+            for name, places in (("mul1", slice(0, T)), ("mul1most", slice(0, T - 1)), ("mul1rest", slice(T - 1, T))):
+                step((name, n), [("e1", i), ("sig1", a)], [("prod1", n)], partial(multiply, places))
             for first in (False, True):
                 step(("turn1", n, first), [("prod1", n)], banks, partial(turn, False, first))
                 step(("mean1", n, first), [("mean1", a)], banks, partial(turn, True, first))
@@ -295,23 +303,26 @@ def tile_gaussian_nn_htanh_v_kernel(
             quantize(("dzn", j, q, g), E5M2, ("dz", k))
             quantize(("dzh", j, q, g), E5M2, ("dzin", k))
 
-        def dx(g, xh, t):
-            bank = ("dxbank", g, xh, t)
-            specs[bank] = ("bank", [P, K], F32)
-            specs["out0", g, xh, t] = ("work", [P, K], F32)
+        def dx(g, xh, t, piece=0, pieces=1):
+            key = (g, xh, t) + (piece,) * (pieces - 1)
+            width = K // pieces
+            bank, out = ("dxbank",) + key, ("out0",) + key
+            specs[bank] = ("bank", [P, width], F32)
+            specs[out] = ("work", [P, width], F32)
             passes = [(q, j) for q in range(2) for j in range(J)]
 
             def multiply(engine):
                 for q, j in passes:
-                    mx(tiles[bank][:], ("dzh", j, q, g), cols(t), E5M2, ("w1", j, xh), cols(q, K), E4M3, (q, j) == passes[0], (q, j) == passes[-1])
+                    columns = cols(pieces * q + piece, width)
+                    mx(tiles[bank][:], ("dzh", j, q, g), cols(t), E5M2, ("w1", j, xh), columns, E4M3, (q, j) == passes[0], (q, j) == passes[-1])
 
             def store(engine):
                 view = out_0.rearrange("(g p t) w -> g p t w", g=2, t=T)[g]
-                engine.dma_start(out=view[:, t, cols(xh, K)], in_=tiles["out0", g, xh, t][:])
+                engine.dma_start(out=view[:, t, cols(pieces * xh + piece, width)], in_=tiles[out][:])
 
-            step(("dx", g, xh, t), [("dzh", j, q, g) for q, j in passes] + [("w1", j, xh) for j in range(J)], [bank], multiply)
-            step(("emptyx", g, xh, t), [bank], [("out0", g, xh, t)], lambda engine: copy(engine, tiles["out0", g, xh, t][:], tiles[bank][:]))
-            step(("store0", g, xh, t), [("out0", g, xh, t)], [], store)
+            step(("dx",) + key, [("dzh", j, q, g) for q, j in passes] + [("w1", j, xh) for j in range(J)], [bank], multiply)
+            step(("emptyx",) + key, [bank], [out], lambda engine: copy(engine, tiles[out][:], tiles[bank][:]))
+            step(("store0",) + key, [out], [], store)
 
         def dw(q, i, j):
             bank = ("dwbank", q, i, j)
@@ -362,6 +373,9 @@ def tile_gaussian_nn_htanh_v_kernel(
                 dx(half, *divmod(k, T))
                 for j in range(J):
                     dw(half, k, j)
+
+        for piece in range(2):
+            dx(1, 1, T - 1, piece, 2)
 
         pe, dve, act, pool, sp = [], [], [], [], []
         inherits = {}
@@ -414,23 +428,23 @@ def tile_gaussian_nn_htanh_v_kernel(
             return means_first(a) + products_first(b)
 
         sp += loads(("sig2", 0), ("e2", 0, 0), ("mu2", 0), ("sig2", 1), ("e2", 0, 1), ("mu2", 1), ("grad", 0, 0), ("e2", 1, 0), ("e2", 1, 1), ("z", 0))
-        sp += loads(("grad", 1, 0), ("sig2", 2), ("e2", 0, 2), ("mu2", 2), ("z", 1), ("sig2", 3), ("e2", 0, 3), ("mu2", 3), ("e2", 1, 2), ("e2", 1, 3))
+        sp += loads(("grad", 1, 0), ("sig2", 2), ("e2", 0, 2), ("mu2", 2), ("z", 1), ("e2", 1, 2))
         sp += loads(("sig1", 0), ("e1", 0), ("mu1", 0), ("z", 2), ("e1", 1), ("sig1", 1), ("e1", 2), ("mu1", 1), ("z", 3), ("grad", 0, 1), ("e1", 3))
-        sp += loads(("x", 0, 0), ("z", 4), ("grad", 1, 1), ("x", 1, 0), ("sig1", 2), ("e1", 4), ("mu1", 2), ("x", 0, 1), ("z", 5), ("x", 1, 1), ("e1", 5))
-        sp += loads(("e1", 6), ("sig1", 3), ("mu1", 3), ("z", 6), ("e1", 7))
+        sp += loads(("sig1", 2), ("e1", 4), ("z", 4), ("mu1", 2), ("grad", 1, 1), ("x", 0, 0), ("z", 5), ("x", 1, 0), ("x", 0, 1), ("e1", 5), ("x", 1, 1))
+        sp += loads(("z", 6), ("sig1", 3), ("e1", 6), ("mu1", 3), ("e1", 7))
         sp += four("store0", 0, 0) + loads(("z", 7))
         pe += products_first(w2(0, 0, "mean2")) + means_first(w2(0, 1, "mean2")) + [("turng", 0, 0)] + around(w2(1, 0, "mean2"), w2(1, 1, "mean2"))
         dve += [("mul2", 0, 0), ("mul2", 0, 1), ("mul2", 1, 0), ("mul2", 1, 1)] + two("emptyg", 0, 0) + quant("w2", 0, 0) + quant("g", 0, 0) + [("empty2", 1, 0, 0)]
         act += [("sort2", 0), ("sort2", 1)] + two("empty2", 0, 0) + two("empty2", 0, 1) + two("abs", 0) + [("empty2", 1, 0, 1)] + two("empty2", 1, 1)
-        pe += four("dh", 0) + [("turng", 1, 0)] + open_with("raw2", 0, 2) + two("turnz", 0) + open_with("raw2", 0, 3) + close_with("turn2", 0, 2) + close_with("turn2", 0, 3)
-        dve += four("mask", 0) + [("mul2", 0, 2)] + dzn(0) + [("mul2", 0, 3)] + quant("w2", 1, 0) + [("mul2", 1, 2)] + quant("g", 1, 0) + [("mul2", 1, 3)] + dzh(0)
-        act += two("emptyg", 1, 0) + [("abs", 1, 0)] + two("emptyz", 0) + [("abs", 1, 1)] + two("empty2", 0, 2) + two("empty2", 0, 3)
-        pe += four("dh", 1) + products_first(w2(1, 2, "raw2"), w2(1, 3, "raw2")) + two("turnz", 1) + around(w1(0), w1(1))
-        dve += four("mask", 1) + [("sort1", 0)] + dzn(1) + [("mul1", 1)] + quant("w2", 0, 1) + [("mul1", 2), ("mul1", 3)] + quant("w2", 1, 1) + [("sort1", 1)] + dzh(1)
-        on_pool(("mul1", 0), ("prod1", 0), ("dzin", 0))
-        act += two("abs", 2) + two("empty2", 1, 2) + two("empty2", 1, 3) + two("emptyz", 1) + two("empty1", 0) + two("empty1", 1)
-        pe += four("dh", 2) + products_first(w1(2), w1(3)) + two("turnz", 2) + open_with("mean1", 4) + [("turng", 0, 1)] + open_with("mean1", 5) + close_with("turn1", 4) + close_with("turn1", 5)
-        dve += four("mask", 2) + two("empty1", 2) + [("mul1", 5)] + dzn(2) + [("mul1", 6)] + two("emptyg", 0, 1) + [("mul1", 7)] + dzh(2)
+        pe += four("dh", 0) + [("turng", 1, 0)] + two("turnz", 0) + four("dh", 1) + products_first(w2(0, 2, "raw2")) + means_first(w2(0, 3, "raw2"))
+        dve += four("mask", 0) + quant("w2", 1, 0) + quant("g", 1, 0) + [("mul2", 0, 2)] + dzn(0) + [("mul2", 0, 3), ("mul2", 1, 2)]
+        act += two("emptyg", 1, 0) + two("emptyz", 0) + two("abs", 1) + two("empty2", 0, 2) + [("empty2", 0, 3, 0)]
+        pe += products_first(w2(1, 2, "raw2")) + two("turnz", 1) + means_first(w2(1, 3, "raw2")) + around(w1(0), w1(1))
+        dve += four("mask", 1) + [("empty2", 0, 3, 1), ("mul1rest", 0), ("mul2", 1, 3), ("sort1", 0)] + dzn(1) + [("mul1", 1)] + quant("w2", 0, 1) + dzh(0) + [("mul1", 2), ("mul1", 3), ("sort1", 1)] + dzh(1)
+        on_pool(("mul1most", 0), ("prod1", 0), ("gin", 1, 0))
+        act += two("empty2", 1, 2) + two("abs", 2) + two("emptyz", 1) + two("empty2", 1, 3) + two("empty1", 0) + two("empty1", 1)
+        pe += four("dh", 2) + around(w1(2), w1(3)) + two("turnz", 2) + open_with("mean1", 4) + [("turng", 0, 1)] + open_with("mean1", 5) + close_with("turn1", 4) + close_with("turn1", 5)
+        dve += four("mask", 2) + two("empty1", 2) + [("mul1", 5)] + quant("w2", 1, 1) + dzn(2) + [("mul1", 6)] + two("emptyg", 0, 1) + [("mul1", 7)] + dzh(2)
         on_pool(("mul1", 4), ("prod1", 4), ("dzin", 1))
         act += two("abs", 3) + two("empty1", 3) + two("emptyz", 2) + two("empty1", 4) + two("empty1", 5)
         pe += four("dh", 3) + around(w1(6), w1(7)) + two("turnz", 3) + open_with("mean1", 8) + [("turng", 1, 1)] + close_with("turn1", 8)
@@ -438,34 +452,40 @@ def tile_gaussian_nn_htanh_v_kernel(
         on_pool(("mul1", 8), ("prod1", 8), ("dzin", 2))
         act += two("abs", 4) + [("empty1", 6, 0)] + two("empty1", 7) + two("emptyz", 3) + two("emptyg", 1, 1)
         pe += four("dh", 4) + [("dx", 0, 0, 0), ("dx", 0, 0, 1)] + two("turnz", 4) + [("dx", 0, 0, 2)] + means_first(w1(9)) + [("dx", 0, 0, 3)]
-        dve += four("mask", 4) + quant("xq", 0, 0) + dzn(4) + quant("g", 1, 1) + two("weave", 1, 0) + two("weave", 0, 1) + quant("xq", 1, 0) + quant("xq", 0, 1) + dzh(4)
-        on_pool(("mul1", 9), ("prod1", 9), ("dzin", 3))
-        act += two("empty1", 8) + two("abs", 5) + [("emptyx", 0, 0, 0), ("emptyx", 0, 0, 1)] + two("emptyz", 4) + [("emptyx", 0, 0, 2)] + two("empty1", 9) + [("emptyx", 0, 0, 3)]
+        dve += four("mask", 4) + [("mul1rest", 9)] + quant("xq", 0, 0) + dzn(4) + quant("g", 1, 1) + two("weave", 1, 0) + two("weave", 0, 1) + quant("xq", 1, 0) + quant("xq", 0, 1) + dzh(4)
+        on_pool(("mul1most", 9), ("prod1", 9), ("dzin", 3))
+        act += two("empty1", 8) + two("abs", 5) + [("emptyx", 0, 0, 0), ("emptyx", 0, 0, 1)] + two("emptyz", 4) + [("emptyx", 0, 0, 2)] + two("empty1", 9)
         pe += four("dh", 5) + dws("dw", 0, 0, range(4)) + two("turnz", 5) + around(w1(10), w1(11)) + dws("dw", 0, 0, range(4, 8))
-        dve += four("mask", 5) + dws("weigh", 0, 0, range(4)) + dzn(5) + quant("xq", 1, 1) + [("sort1", 3), ("mul1", 12)] + dzh(5) + dws("weigh", 0, 0, range(4, 8))
+        dve += four("mask", 5) + dws("weigh", 0, 0, range(4)) + [("mul1rest", 11)] + dzn(5) + quant("xq", 1, 1) + [("sort1", 3), ("mul1", 12)] + dzh(5) + dws("weigh", 0, 0, range(4, 8))
         on_pool(("mul1", 10), ("prod1", 10), ("dzin", 4))
-        pool.append(("mul1", 11))
-        act += two("weave", 1, 1) + two("emptyz", 5) + two("abs", 6) + two("empty1", 10) + two("empty1", 11)
+        pool.append(("mul1most", 11))
+        act += [("emptyx", 0, 0, 3)] + two("weave", 1, 1) + two("emptyz", 5) + two("abs", 6) + two("empty1", 10) + two("empty1", 11)
         pe += four("dh", 6) + around(w1(12), w1(13)) + two("turnz", 6) + dws("dw", 0, 1, range(8))
-        dve += four("mask", 6) + [("mul1", 15)] + dzn(6) + dws("weigh", 0, 1, range(8))
+        dve += four("mask", 6) + [("mul1rest", 14)] + dzn(6) + [("mul1", 15)] + dws("weigh", 0, 1, range(8))
         on_pool(("mul1", 13), ("prod1", 13), ("dzin", 5))
-        pool += [("mul1", 14)]
+        pool += [("mul1most", 14)]
         act += two("abs", 7) + two("empty1", 12) + two("empty1", 13) + two("emptyz", 6)
         pe += four("dh", 7) + dws("dw", 1, 0, range(4)) + two("turnz", 7) + dws("dw", 1, 0, range(4, 8))
-        dve += four("mask", 7) + dws("weigh", 1, 0, range(4)) + dzn(7) + dzh(6) + dzh(7) + dws("weigh", 1, 0, range(4, 8))
+        dve += four("mask", 7) + dws("weigh", 1, 0, range(4)) + dzh(6) + dzn(7) + dzh(7) + [("add1", 14), ("add1", 15)]
         pool += four("sum", 0)[:3]
-        on_pool(("sum", 0, 3), ("total", 0, 3), ("dzin", 7))
         act += two("emptyz", 7)
         sp += four("store1", 0)[:3]
-        pe += four("dx", 1, 0)[:3] + [("turn1w", 14), ("turn1w", 15), ("dx", 1, 0, 3)] + dws("dw", 1, 1, range(8))
-        pe += four("dx", 0, 1) + four("dx", 1, 1)
-        dve += [("add1", 14), ("add1", 15)] + quant("w1", 0, 1) + quant("w1", 1, 1) + dws("weigh", 1, 1, range(8)) + four("sum", 1)[1:]
-        pool.append(("sum", 1, 0))
-        act += four("emptyx", 1, 0)[:3] + [("empty1w", 14), ("empty1w", 15), ("emptyx", 1, 0, 3)] + four("emptyx", 0, 1) + four("emptyx", 1, 1)
-        sp += [("store0", 1, 0, 0), ("store1", 0, 3)] + four("store0", 1, 0)[1:]
+        pe += four("dx", 1, 0)[:2] + [("turn1w", 14), ("dx", 1, 0, 2), ("turn1w", 15), ("dx", 1, 0, 3)]
+        dve += dws("weigh", 1, 0, range(4, 8)) + quant("w1", 0, 1) + quant("w1", 1, 1)
+        act += four("emptyx", 1, 0)[:2] + [("empty1w", 14), ("emptyx", 1, 0, 2), ("empty1w", 15), ("emptyx", 1, 0, 3)]
+        pe += dws("dw", 1, 1, range(4))
         for n in range(T):
-            sp += [("store1", 1, n), ("store0", 0, 1, n)]
-        sp += four("store0", 1, 1)
+            pe += dws("dw", 1, 1, range(8)[4 + 2 * n : 6 + 2 * n]) + [("dx", 0, 1, n)]
+        pe += four("dx", 1, 1)[:3] + two("dx", 1, 1, 3)
+        dve += dws("weigh", 1, 1, range(6)) + [("sum", 1, 1), ("sum", 1, 2)] + dws("weigh", 1, 1, range(6, 8)) + [("sum", 1, 3)]
+        pool += [("sum", 0, 3), ("sum", 1, 0)]
+        inherits["total", 0, 3] = ("prod1", 15)
+        act += four("emptyx", 0, 1) + four("emptyx", 1, 1)[:3] + [("emptyx", 1, 1, 3, 0)]
+        dve.append(("emptyx", 1, 1, 3, 1))
+        sp += four("store0", 1, 0)[:2] + [("store1", 0, 3)] + four("store0", 1, 0)[2:]
+        for n in range(T):
+            sp += [("store0", 0, 1, n), ("store1", 1, n)]
+        sp += four("store0", 1, 1)[:3] + two("store0", 1, 1, 3)
 
 
         queues = [(nc.tensor, pe), (nc.vector, dve), (nc.scalar, act), (nc.gpsimd, pool), (nc.sync, sp)]
@@ -495,8 +515,8 @@ def tile_gaussian_nn_htanh_v_kernel(
         def take(key):
             kind, shape, dtype = specs[key]
             if key not in inherits:
-                slots[key] = free[kind].pop(0)
-            tag = "%s%d" % (kind, slots[key])
+                slots[key] = (kind, free[kind].pop(0))
+            tag = "%s%d" % slots[key]
             if kind == "bank":
                 tiles[key] = psum.tile(shape, dtype, name=key[0], tag=tag)
             elif kind in ("code", "wide"):
@@ -518,7 +538,7 @@ def tile_gaussian_nn_htanh_v_kernel(
                 if readers[key] == 0 and key in heirs:
                     slots[heirs[key]] = slots[key]
                 elif readers[key] == 0 and key in specs:
-                    free[specs[key][0]].append(slots[key])
+                    free[slots[key][0]].append(slots[key][1])
 
         while any(queue for engine, queue in queues):
             heads = [(engine, queue) for engine, queue in queues if queue and ready(queue[0])]

@@ -131,9 +131,9 @@ def tile_gaussian_nn_htanh_v_kernel(
             banks = banks_for(("w2bank", j, a), 2, [P, T, P])
 
             def multiply(engine):
-                walk = "p b (w i t) -> p (b w) t i"
+                walk, order = ("p b (w i t) -> p (b w) t i", "p t b (w i) -> p (b w) t i") if engine is nc.vector else ("p b (w i t) -> p t (b w i)", "p t b (w i) -> p t (b w i)")
                 engine.tensor_tensor(
-                    out=tiles["prod2", j, a][:].rearrange("p t b (w i) -> p (b w) t i", i=2),
+                    out=tiles["prod2", j, a][:].rearrange(order, i=2),
                     in0=w2_in(("e2", j), a).rearrange(walk, t=T, i=2),
                     in1=w2_in(("sig2",), a).rearrange(walk, t=T, i=2),
                     op=ALU.mult,
@@ -249,7 +249,7 @@ def tile_gaussian_nn_htanh_v_kernel(
                 dst = tiles["w1in", j, xh][:].rearrange("p c t -> p (c t)").bitcast(F32).rearrange("p (q c m s) -> p q c m s", q=2, m=P, s=2)
                 copy(engine, dst[:, :, c], tiles["w1words", n][:].rearrange("p q s m -> p q m s"))
 
-            for name, places in (("mul1", slice(0, T)), ("mul1most", slice(0, T - 1)), ("mul1rest", slice(T - 1, T))):
+            for name, places in (("mul1", slice(0, T)), ("mul1most", slice(0, T - 1)), ("mul1rest", slice(T - 1, T)), ("mul1low", slice(0, 2)), ("mul1high", slice(2, T))):
                 step((name, n), [("e1", i), ("sig1", a)], [("prod1", n)], partial(multiply, places))
             for first in (False, True):
                 step(("turn1", n, first), [("prod1", n)], banks, partial(turn, False, first))
@@ -263,7 +263,8 @@ def tile_gaussian_nn_htanh_v_kernel(
 
         def unit(k):
             j, q, g = UNITS[k]
-            load(("z", k), "z", [P, T, K], F32, z1[j].rearrange("(g p t) h -> g p t h", g=2, t=T)[g][:, :, cols(q, K)])
+            rows = z1[j].rearrange("(g p t) h -> g p t h", g=2, t=T)[g]
+            load(("z", k), "z", [P, T, K], F32, rows[:, :, cols(q, K)])
             for name in ("abs", "dz", "dzin"):
                 specs[name, k] = ("work", [P, K, T], BF16)
             dh = banks_for(("dhbank", k), T, [P, T, P])
@@ -284,8 +285,11 @@ def tile_gaussian_nn_htanh_v_kernel(
                 bank = tiles[dh[u]][:].rearrange("p t (b i) -> p b i t", i=RUN)
                 engine.scalar_tensor_tensor(out=dz[:, u], in0=size[:, u], scalar=EDGE, in1=bank, op0=ALU.is_lt, op1=ALU.mult)
 
-            def turn(s, engine):
-                words = tiles["dz", k][:].rearrange("p c t -> p (c t)").bitcast(F32).rearrange("p (u m s) -> p s u m", u=T, s=2)
+            def words_of(name):
+                return tiles[name, k][:].rearrange("p c t -> p (c t)").bitcast(F32)
+
+            def turn(s, source, engine):
+                words = words_of(source).rearrange("p (u m s) -> p s u m", u=T, s=2)
                 for u in range(T):
                     engine.transpose(tiles[turned[s]][:, u, :], words[:, s, u, :], ident_f[:])
 
@@ -295,7 +299,7 @@ def tile_gaussian_nn_htanh_v_kernel(
 
             for n in range(2):
                 step(("abs", k, n), [("z", k)], [("abs", k)], partial(absolute, n))
-                step(("turnz", k, n), [("dz", k)], [turned[n]], partial(turn, n))
+                step(("turnz", k, n), [("dz", k)], [turned[n]], partial(turn, n, "dz"))
                 step(("emptyz", k, n), [turned[n]], [("dzin", k)], partial(empty, n))
             for u in range(T):
                 step(("dh", k, u), [("g", j, g), ("w2", j, q)], [dh[u]], partial(multiply, u))
@@ -438,19 +442,19 @@ def tile_gaussian_nn_htanh_v_kernel(
         act += [("sort2", 0), ("sort2", 1)] + two("empty2", 0, 0) + two("empty2", 0, 1) + two("abs", 0) + [("empty2", 1, 0, 1)] + two("empty2", 1, 1)
         pe += four("dh", 0) + [("turng", 1, 0)] + two("turnz", 0) + four("dh", 1) + products_first(w2(0, 2, "raw2")) + means_first(w2(0, 3, "raw2"))
         dve += four("mask", 0) + quant("w2", 1, 0) + quant("g", 1, 0) + [("mul2", 0, 2)] + dzn(0) + [("mul2", 0, 3), ("mul2", 1, 2)]
-        act += two("emptyg", 1, 0) + two("emptyz", 0) + two("abs", 1) + two("empty2", 0, 2) + [("empty2", 0, 3, 0)]
+        act += two("emptyg", 1, 0) + two("emptyz", 0) + two("abs", 1) + two("empty2", 0, 2) + two("empty2", 0, 3)
         pe += products_first(w2(1, 2, "raw2")) + two("turnz", 1) + means_first(w2(1, 3, "raw2")) + around(w1(0), w1(1))
-        dve += four("mask", 1) + [("empty2", 0, 3, 1), ("mul1rest", 0), ("mul2", 1, 3), ("sort1", 0)] + dzn(1) + [("mul1", 1)] + quant("w2", 0, 1) + dzh(0) + [("mul1", 2), ("mul1", 3), ("sort1", 1)] + dzh(1)
+        dve += four("mask", 1) + [("mul1rest", 0), ("mul2", 1, 3), ("sort1", 0)] + dzn(1) + [("mul1", 1)] + quant("w2", 0, 1) + dzh(0) + [("mul1", 2), ("mul1", 3), ("sort1", 1)] + dzh(1)
         on_pool(("mul1most", 0), ("prod1", 0), ("gin", 1, 0))
         act += two("empty2", 1, 2) + two("abs", 2) + two("emptyz", 1) + two("empty2", 1, 3) + two("empty1", 0) + two("empty1", 1)
         pe += four("dh", 2) + around(w1(2), w1(3)) + two("turnz", 2) + open_with("mean1", 4) + [("turng", 0, 1)] + open_with("mean1", 5) + close_with("turn1", 4) + close_with("turn1", 5)
-        dve += four("mask", 2) + two("empty1", 2) + [("mul1", 5)] + quant("w2", 1, 1) + dzn(2) + [("mul1", 6)] + two("emptyg", 0, 1) + [("mul1", 7)] + dzh(2)
+        dve += four("mask", 2) + two("empty1", 2) + [("mul1", 5)] + quant("w2", 1, 1) + dzn(2) + [("mul1", 6), ("mul1", 7)] + dzh(2)
         on_pool(("mul1", 4), ("prod1", 4), ("dzin", 1))
-        act += two("abs", 3) + two("empty1", 3) + two("emptyz", 2) + two("empty1", 4) + two("empty1", 5)
+        act += two("abs", 3) + two("empty1", 3) + two("emptyz", 2) + two("emptyg", 0, 1) + two("empty1", 4) + two("empty1", 5)
         pe += four("dh", 3) + around(w1(6), w1(7)) + two("turnz", 3) + open_with("mean1", 8) + [("turng", 1, 1)] + close_with("turn1", 8)
-        dve += four("mask", 3) + [("empty1", 6, 1), ("sort1", 2)] + dzn(3) + quant("g", 0, 1) + quant("w1", 0, 0) + two("weave", 0, 0) + quant("w1", 1, 0) + dzh(3)
+        dve += four("mask", 3) + [("sort1", 2)] + dzn(3) + quant("g", 0, 1) + quant("w1", 0, 0) + two("weave", 0, 0) + quant("w1", 1, 0) + dzh(3)
         on_pool(("mul1", 8), ("prod1", 8), ("dzin", 2))
-        act += two("abs", 4) + [("empty1", 6, 0)] + two("empty1", 7) + two("emptyz", 3) + two("emptyg", 1, 1)
+        act += two("abs", 4) + two("empty1", 6) + two("empty1", 7) + two("emptyz", 3) + two("emptyg", 1, 1)
         pe += four("dh", 4) + [("dx", 0, 0, 0), ("dx", 0, 0, 1)] + two("turnz", 4) + [("dx", 0, 0, 2)] + means_first(w1(9)) + [("dx", 0, 0, 3)]
         dve += four("mask", 4) + [("mul1rest", 9)] + quant("xq", 0, 0) + dzn(4) + quant("g", 1, 1) + two("weave", 1, 0) + two("weave", 0, 1) + quant("xq", 1, 0) + quant("xq", 0, 1) + dzh(4)
         on_pool(("mul1most", 9), ("prod1", 9), ("dzin", 3))

@@ -182,12 +182,13 @@ def tile_gaussian_nn_htanh_v_kernel(
             load(("x", g, xh), "load", [P, T, K], BF16, x.rearrange("(g p t) w -> g p t w", g=2, t=T)[g][:, :, cols(xh, K)])
             specs["xin", g, xh] = ("work", [P, K, T], BF16)
 
-            def interleave(n, engine):
-                src = tiles["x", g, xh][:, :, cols(n, K // 2)].rearrange("p t (c i) -> p c t i", i=4)
-                copy(engine, tiles["xin", g, xh][:, cols(n, K // 2), :].rearrange("p (c i) t -> p c t i", i=4), src)
+            def interleave(part, engine):
+                src = tiles["x", g, xh][:, :, part].rearrange("p t (c i) -> p c t i", i=4)
+                copy(engine, tiles["xin", g, xh][:, part, :].rearrange("p (c i) t -> p c t i", i=4), src)
 
             for n in range(2):
-                step(("weave", g, xh, n), [("x", g, xh)], [("xin", g, xh)], partial(interleave, n))
+                step(("weave", g, xh, n), [("x", g, xh)], [("xin", g, xh)], partial(interleave, cols(n, K // 2)))
+            step(("weave", g, xh), [("x", g, xh)], [("xin", g, xh)], partial(interleave, cols(0, K)))
             quantize(("xq", g, xh), E4M3, ("xin", g, xh))
 
         def w1_pair(a):
@@ -354,14 +355,16 @@ def tile_gaussian_nn_htanh_v_kernel(
             first, second, total = ("part", q, a, 0), ("part", q, a, 1), ("total", q, a)
             specs[total] = ("work", [P, 2, K], F32)
 
-            def add(engine):
-                engine.tensor_tensor(out=tiles[total][:], in0=tiles[first][:], in1=tiles[second][:], op=ALU.add)
+            def add(rows, engine):
+                engine.tensor_tensor(out=tiles[total][:, rows], in0=tiles[first][:, rows], in1=tiles[second][:, rows], op=ALU.add)
 
             def store(engine):
                 view = out_1.rearrange("(a r m) h -> a m r h", r=2, m=P)[a][:, :, cols(q, K)]
                 engine.dma_start(out=view, in_=tiles[total][:])
 
-            step(("sum", q, a), [first, second], [total], add)
+            step(("sum", q, a), [first, second], [total], partial(add, slice(0, 2)))
+            for r in range(2):
+                step(("sum", q, a, r), [first, second], [total], partial(add, slice(r, r + 1)))
             step(("store1", q, a), [total], [], store)
 
         for a in range(4):
@@ -434,8 +437,8 @@ def tile_gaussian_nn_htanh_v_kernel(
         sp += loads(("sig2", 0), ("e2", 0, 0), ("mu2", 0), ("sig2", 1), ("e2", 0, 1), ("mu2", 1), ("grad", 0, 0), ("e2", 1, 0), ("e2", 1, 1), ("z", 0))
         sp += loads(("grad", 1, 0), ("sig2", 2), ("e2", 0, 2), ("mu2", 2), ("z", 1), ("e2", 1, 2))
         sp += loads(("sig1", 0), ("e1", 0), ("mu1", 0), ("z", 2), ("e1", 1), ("sig1", 1), ("e1", 2), ("mu1", 1), ("z", 3), ("grad", 0, 1), ("e1", 3))
-        sp += loads(("sig1", 2), ("e1", 4), ("z", 4), ("mu1", 2), ("grad", 1, 1), ("x", 0, 0), ("z", 5), ("x", 1, 0), ("x", 0, 1), ("e1", 5), ("x", 1, 1))
-        sp += loads(("z", 6), ("sig1", 3), ("e1", 6), ("mu1", 3), ("e1", 7))
+        sp += loads(("sig1", 2), ("e1", 4), ("z", 4), ("mu1", 2), ("grad", 1, 1), ("x", 0, 0), ("z", 5), ("x", 1, 0), ("mu1", 3), ("e1", 5), ("x", 1, 1))
+        sp += loads(("z", 6), ("sig1", 3), ("e1", 6), ("x", 0, 1), ("e1", 7))
         sp += four("store0", 0, 0) + loads(("z", 7))
         pe += products_first(w2(0, 0, "mean2")) + means_first(w2(0, 1, "mean2")) + [("turng", 0, 0)] + around(w2(1, 0, "mean2"), w2(1, 1, "mean2"))
         dve += [("mul2", 0, 0), ("mul2", 0, 1), ("mul2", 1, 0), ("mul2", 1, 1)] + two("emptyg", 0, 0) + quant("w2", 0, 0) + quant("g", 0, 0) + [("empty2", 1, 0, 0)]
@@ -452,26 +455,27 @@ def tile_gaussian_nn_htanh_v_kernel(
         on_pool(("mul1", 4), ("prod1", 4), ("dzin", 1))
         act += two("abs", 3) + two("empty1", 3) + two("emptyz", 2) + two("emptyg", 0, 1) + two("empty1", 4) + two("empty1", 5)
         pe += four("dh", 3) + around(w1(6), w1(7)) + two("turnz", 3) + open_with("mean1", 8) + [("turng", 1, 1)] + close_with("turn1", 8)
-        dve += four("mask", 3) + [("sort1", 2)] + dzn(3) + quant("g", 0, 1) + quant("w1", 0, 0) + two("weave", 0, 0) + quant("w1", 1, 0) + dzh(3)
-        on_pool(("mul1", 8), ("prod1", 8), ("dzin", 2))
+        dve += four("mask", 3) + [("mul1rest", 8), ("sort1", 2)] + dzn(3) + quant("g", 0, 1) + quant("w1", 0, 0) + [("weave", 0, 0)] + quant("w1", 1, 0) + dzh(3)
+        on_pool(("mul1most", 8), ("prod1", 8), ("dzin", 2))
         act += two("abs", 4) + two("empty1", 6) + two("empty1", 7) + two("emptyz", 3) + two("emptyg", 1, 1)
         pe += four("dh", 4) + [("dx", 0, 0, 0), ("dx", 0, 0, 1)] + two("turnz", 4) + [("dx", 0, 0, 2)] + means_first(w1(9)) + [("dx", 0, 0, 3)]
-        dve += four("mask", 4) + [("mul1rest", 9)] + quant("xq", 0, 0) + dzn(4) + quant("g", 1, 1) + two("weave", 1, 0) + two("weave", 0, 1) + quant("xq", 1, 0) + quant("xq", 0, 1) + dzh(4)
+        dve += four("mask", 4) + [("mul1rest", 9)] + quant("xq", 0, 0) + dzn(4) + quant("g", 1, 1) + [("weave", 1, 0), ("sort1", 3)] + quant("xq", 1, 0) + dzh(4)
         on_pool(("mul1most", 9), ("prod1", 9), ("dzin", 3))
         act += two("empty1", 8) + two("abs", 5) + [("emptyx", 0, 0, 0), ("emptyx", 0, 0, 1)] + two("emptyz", 4) + [("emptyx", 0, 0, 2)] + two("empty1", 9)
-        pe += four("dh", 5) + dws("dw", 0, 0, range(4)) + two("turnz", 5) + around(w1(10), w1(11)) + dws("dw", 0, 0, range(4, 8))
-        dve += four("mask", 5) + dws("weigh", 0, 0, range(4)) + [("mul1rest", 11)] + dzn(5) + quant("xq", 1, 1) + [("sort1", 3), ("mul1", 12)] + dzh(5) + dws("weigh", 0, 0, range(4, 8))
+        pe += four("dh", 5) + dws("dw", 0, 0, range(4)) + two("turnz", 5) + around(w1(10), w1(11)) + dws("dw", 0, 1, range(4))
+        dve += four("mask", 5) + dws("weigh", 0, 0, range(4)) + [("mul1rest", 11)] + dzn(5) + [("mul1", 12)] + dzh(5) + dws("weigh", 0, 1, range(4))
         on_pool(("mul1", 10), ("prod1", 10), ("dzin", 4))
         pool.append(("mul1most", 11))
         act += [("emptyx", 0, 0, 3)] + two("weave", 1, 1) + two("emptyz", 5) + two("abs", 6) + two("empty1", 10) + two("empty1", 11)
-        pe += four("dh", 6) + around(w1(12), w1(13)) + two("turnz", 6) + dws("dw", 0, 1, range(8))
-        dve += four("mask", 6) + [("mul1rest", 14)] + dzn(6) + [("mul1", 15)] + dws("weigh", 0, 1, range(8))
+        pe += four("dh", 6) + around(w1(12), w1(13)) + two("turnz", 6) + dws("dw", 0, 0, range(4, 8)) + dws("dw", 0, 1, range(4, 8))
+        dve += four("mask", 6) + [("mul1rest", 14)] + quant("xq", 1, 1) + quant("xq", 0, 1) + dzn(6) + [("mul1", 15)] + dws("weigh", 0, 0, range(4, 8)) + dws("weigh", 0, 1, range(4, 8))
         on_pool(("mul1", 13), ("prod1", 13), ("dzin", 5))
         pool += [("mul1most", 14)]
-        act += two("abs", 7) + two("empty1", 12) + two("empty1", 13) + two("emptyz", 6)
+        act += two("weave", 0, 1) + two("empty1", 12) + two("empty1", 13) + two("emptyz", 6) + two("abs", 7)
         pe += four("dh", 7) + dws("dw", 1, 0, range(4)) + two("turnz", 7) + dws("dw", 1, 0, range(4, 8))
         dve += four("mask", 7) + dws("weigh", 1, 0, range(4)) + dzh(6) + dzn(7) + dzh(7) + [("add1", 14), ("add1", 15)]
-        pool += four("sum", 0)[:3]
+        on_pool(("sum", 0, 0), ("total", 0, 0), ("sig1", 3))
+        pool += [("sum", 0, 1), ("sum", 0, 2)]
         act += two("emptyz", 7)
         sp += four("store1", 0)[:3]
         pe += four("dx", 1, 0)[:2] + [("turn1w", 14), ("dx", 1, 0, 2), ("turn1w", 15), ("dx", 1, 0, 3)]
@@ -479,7 +483,7 @@ def tile_gaussian_nn_htanh_v_kernel(
         act += four("emptyx", 1, 0)[:2] + [("empty1w", 14), ("emptyx", 1, 0, 2), ("empty1w", 15), ("emptyx", 1, 0, 3)]
         pe += dws("dw", 1, 1, range(4))
         for n in range(T):
-            pe += dws("dw", 1, 1, range(8)[4 + 2 * n : 6 + 2 * n]) + [("dx", 0, 1, n)]
+            pe += [("dx", 0, 1, n)] + dws("dw", 1, 1, range(8)[4 + 2 * n : 6 + 2 * n])
         pe += four("dx", 1, 1)[:3] + two("dx", 1, 1, 3)
         dve += dws("weigh", 1, 1, range(6)) + [("sum", 1, 1), ("sum", 1, 2)] + dws("weigh", 1, 1, range(6, 8)) + [("sum", 1, 3)]
         pool += [("sum", 0, 3), ("sum", 1, 0)]

@@ -458,24 +458,24 @@ def tile_gaussian_nn_htanh_v_kernel(
         dve += four("mask", 3) + [("mul1rest", 8), ("sort1", 2)] + dzn(3) + quant("g", 0, 1) + quant("w1", 0, 0) + [("weave", 0, 0)] + quant("w1", 1, 0) + dzh(3)
         on_pool(("mul1most", 8), ("prod1", 8), ("dzin", 2))
         act += two("abs", 4) + two("empty1", 6) + two("empty1", 7) + two("emptyz", 3) + two("emptyg", 1, 1)
-        pe += four("dh", 4) + [("dx", 0, 0, 0), ("dx", 0, 0, 1)] + two("turnz", 4) + [("dx", 0, 0, 2)] + means_first(w1(9)) + [("dx", 0, 0, 3)]
+        pe += four("dh", 4) + four("dx", 0, 0)[:3] + two("turnz", 4) + means_first(w1(9)) + [("dx", 0, 0, 3)]
         dve += four("mask", 4) + [("mul1rest", 9)] + quant("xq", 0, 0) + dzn(4) + quant("g", 1, 1) + [("weave", 1, 0), ("sort1", 3)] + quant("xq", 1, 0) + dzh(4)
         on_pool(("mul1most", 9), ("prod1", 9), ("dzin", 3))
-        act += two("empty1", 8) + two("abs", 5) + [("emptyx", 0, 0, 0), ("emptyx", 0, 0, 1)] + two("emptyz", 4) + [("emptyx", 0, 0, 2)] + two("empty1", 9)
+        act += two("empty1", 8) + two("abs", 5) + four("emptyx", 0, 0)[:3] + two("emptyz", 4) + two("empty1", 9)
         pe += four("dh", 5) + dws("dw", 0, 0, range(4)) + two("turnz", 5) + around(w1(10), w1(11)) + dws("dw", 0, 1, range(4))
         dve += four("mask", 5) + dws("weigh", 0, 0, range(4)) + [("mul1rest", 11)] + dzn(5) + [("mul1", 12)] + dzh(5) + dws("weigh", 0, 1, range(4))
         on_pool(("mul1", 10), ("prod1", 10), ("dzin", 4))
         pool.append(("mul1most", 11))
         act += [("emptyx", 0, 0, 3)] + two("weave", 1, 1) + two("emptyz", 5) + two("abs", 6) + two("empty1", 10) + two("empty1", 11)
         pe += four("dh", 6) + around(w1(12), w1(13)) + two("turnz", 6) + dws("dw", 0, 0, range(4, 8)) + dws("dw", 0, 1, range(4, 8))
-        dve += four("mask", 6) + [("mul1rest", 14)] + quant("xq", 1, 1) + quant("xq", 0, 1) + dzn(6) + [("mul1", 15)] + dws("weigh", 0, 0, range(4, 8)) + dws("weigh", 0, 1, range(4, 8))
+        dve += four("mask", 6) + [("mul1rest", 14)] + quant("xq", 1, 1) + quant("xq", 0, 1) + [("mul1high", 15)] + dzn(6) + dws("weigh", 0, 0, range(4, 8)) + dws("weigh", 0, 1, range(4, 8))
         on_pool(("mul1", 13), ("prod1", 13), ("dzin", 5))
         pool += [("mul1most", 14)]
         act += two("weave", 0, 1) + two("empty1", 12) + two("empty1", 13) + two("emptyz", 6) + two("abs", 7)
         pe += four("dh", 7) + dws("dw", 1, 0, range(4)) + two("turnz", 7) + dws("dw", 1, 0, range(4, 8))
         dve += four("mask", 7) + dws("weigh", 1, 0, range(4)) + dzh(6) + dzn(7) + dzh(7) + [("add1", 14), ("add1", 15)]
-        on_pool(("sum", 0, 0), ("total", 0, 0), ("sig1", 3))
-        pool += [("sum", 0, 1), ("sum", 0, 2)]
+        on_pool(("sum", 0, 0), ("total", 0, 0), ("dz", 6))
+        pool += [("sum", 0, 1), ("sum", 0, 2), ("mul1low", 15)]
         act += two("emptyz", 7)
         sp += four("store1", 0)[:3]
         pe += four("dx", 1, 0)[:2] + [("turn1w", 14), ("dx", 1, 0, 2), ("turn1w", 15), ("dx", 1, 0, 3)]

@@ -58,10 +58,8 @@ def tile_gaussian_nn_htanh_v_kernel(
         def copy(engine, out, in_):
             if engine is nc.scalar:
                 nc.scalar.copy(out=out, in_=in_)
-            elif engine is nc.vector:
-                nc.vector.tensor_copy(out=out, in_=in_)
             else:
-                nc.gpsimd.tensor_scalar(out=out, in0=in_, scalar1=1.0, scalar2=0.0, op0=ALU.mult, op1=ALU.add)
+                nc.vector.tensor_copy(out=out, in_=in_)
 
         def load(key, kind, shape, dtype, src):
             specs[key] = (kind, shape, dtype)
@@ -131,9 +129,9 @@ def tile_gaussian_nn_htanh_v_kernel(
             banks = banks_for(("w2bank", j, a), 2, [P, T, P])
 
             def multiply(engine):
-                walk, order = ("p b (w i t) -> p (b w) t i", "p t b (w i) -> p (b w) t i") if engine is nc.vector else ("p b (w i t) -> p t (b w i)", "p t b (w i) -> p t (b w i)")
+                walk = "p b (w i t) -> p (b w) t i"
                 engine.tensor_tensor(
-                    out=tiles["prod2", j, a][:].rearrange(order, i=2),
+                    out=tiles["prod2", j, a][:].rearrange("p t b (w i) -> p (b w) t i", i=2),
                     in0=w2_in(("e2", j), a).rearrange(walk, t=T, i=2),
                     in1=w2_in(("sig2",), a).rearrange(walk, t=T, i=2),
                     op=ALU.mult,
@@ -250,8 +248,9 @@ def tile_gaussian_nn_htanh_v_kernel(
                 dst = tiles["w1in", j, xh][:].rearrange("p c t -> p (c t)").bitcast(F32).rearrange("p (q c m s) -> p q c m s", q=2, m=P, s=2)
                 copy(engine, dst[:, :, c], tiles["w1words", n][:].rearrange("p q s m -> p q m s"))
 
-            for name, places in (("mul1", slice(0, T)), ("mul1most", slice(0, T - 1)), ("mul1rest", slice(T - 1, T)), ("mul1low", slice(0, 2)), ("mul1high", slice(2, T))):
-                step((name, n), [("e1", i), ("sig1", a)], [("prod1", n)], partial(multiply, places))
+            shares = {"mul1": (0, T), "mul1most": (0, T - 1), "mul1rest": (T - 1, T), "mul1low": (0, 2), "mul1high": (2, T)}
+            for name, places in shares.items():
+                step((name, n), [("e1", i), ("sig1", a)], [("prod1", n)], partial(multiply, slice(*places)))
             for first in (False, True):
                 step(("turn1", n, first), [("prod1", n)], banks, partial(turn, False, first))
                 step(("mean1", n, first), [("mean1", a)], banks, partial(turn, True, first))
@@ -264,8 +263,7 @@ def tile_gaussian_nn_htanh_v_kernel(
 
         def unit(k):
             j, q, g = UNITS[k]
-            rows = z1[j].rearrange("(g p t) h -> g p t h", g=2, t=T)[g]
-            load(("z", k), "z", [P, T, K], F32, rows[:, :, cols(q, K)])
+            load(("z", k), "z", [P, T, K], F32, z1[j].rearrange("(g p t) h -> g p t h", g=2, t=T)[g][:, :, cols(q, K)])
             for name in ("abs", "dz", "dzin"):
                 specs[name, k] = ("work", [P, K, T], BF16)
             dh = banks_for(("dhbank", k), T, [P, T, P])
@@ -286,11 +284,8 @@ def tile_gaussian_nn_htanh_v_kernel(
                 bank = tiles[dh[u]][:].rearrange("p t (b i) -> p b i t", i=RUN)
                 engine.scalar_tensor_tensor(out=dz[:, u], in0=size[:, u], scalar=EDGE, in1=bank, op0=ALU.is_lt, op1=ALU.mult)
 
-            def words_of(name):
-                return tiles[name, k][:].rearrange("p c t -> p (c t)").bitcast(F32)
-
-            def turn(s, source, engine):
-                words = words_of(source).rearrange("p (u m s) -> p s u m", u=T, s=2)
+            def turn(s, engine):
+                words = tiles["dz", k][:].rearrange("p c t -> p (c t)").bitcast(F32).rearrange("p (u m s) -> p s u m", u=T, s=2)
                 for u in range(T):
                     engine.transpose(tiles[turned[s]][:, u, :], words[:, s, u, :], ident_f[:])
 
@@ -300,7 +295,7 @@ def tile_gaussian_nn_htanh_v_kernel(
 
             for n in range(2):
                 step(("abs", k, n), [("z", k)], [("abs", k)], partial(absolute, n))
-                step(("turnz", k, n), [("dz", k)], [turned[n]], partial(turn, n, "dz"))
+                step(("turnz", k, n), [("dz", k)], [turned[n]], partial(turn, n))
                 step(("emptyz", k, n), [turned[n]], [("dzin", k)], partial(empty, n))
             for u in range(T):
                 step(("dh", k, u), [("g", j, g), ("w2", j, q)], [dh[u]], partial(multiply, u))
@@ -355,16 +350,14 @@ def tile_gaussian_nn_htanh_v_kernel(
             first, second, total = ("part", q, a, 0), ("part", q, a, 1), ("total", q, a)
             specs[total] = ("work", [P, 2, K], F32)
 
-            def add(rows, engine):
-                engine.tensor_tensor(out=tiles[total][:, rows], in0=tiles[first][:, rows], in1=tiles[second][:, rows], op=ALU.add)
+            def add(engine):
+                engine.tensor_tensor(out=tiles[total][:], in0=tiles[first][:], in1=tiles[second][:], op=ALU.add)
 
             def store(engine):
                 view = out_1.rearrange("(a r m) h -> a m r h", r=2, m=P)[a][:, :, cols(q, K)]
                 engine.dma_start(out=view, in_=tiles[total][:])
 
-            step(("sum", q, a), [first, second], [total], partial(add, slice(0, 2)))
-            for r in range(2):
-                step(("sum", q, a, r), [first, second], [total], partial(add, slice(r, r + 1)))
+            step(("sum", q, a), [first, second], [total], add)
             step(("store1", q, a), [total], [], store)
 
         for a in range(4):
@@ -380,13 +373,11 @@ def tile_gaussian_nn_htanh_v_kernel(
                 dx(half, *divmod(k, T))
                 for j in range(J):
                     dw(half, k, j)
-
         for piece in range(2):
             dx(1, 1, T - 1, piece, 2)
 
         pe, dve, act, pool, sp = [], [], [], [], []
         inherits = {}
-
 
         def two(*name):
             return [name + (0,), name + (1,)]
@@ -446,6 +437,7 @@ def tile_gaussian_nn_htanh_v_kernel(
         pe += four("dh", 0) + [("turng", 1, 0)] + two("turnz", 0) + four("dh", 1) + products_first(w2(0, 2, "raw2")) + means_first(w2(0, 3, "raw2"))
         dve += four("mask", 0) + quant("w2", 1, 0) + quant("g", 1, 0) + [("mul2", 0, 2)] + dzn(0) + [("mul2", 0, 3), ("mul2", 1, 2)]
         act += two("emptyg", 1, 0) + two("emptyz", 0) + two("abs", 1) + two("empty2", 0, 2) + two("empty2", 0, 3)
+
         pe += products_first(w2(1, 2, "raw2")) + two("turnz", 1) + means_first(w2(1, 3, "raw2")) + around(w1(0), w1(1))
         dve += four("mask", 1) + [("mul1rest", 0), ("mul2", 1, 3), ("sort1", 0)] + dzn(1) + [("mul1", 1)] + quant("w2", 0, 1) + dzh(0) + [("mul1", 2), ("mul1", 3), ("sort1", 1)] + dzh(1)
         on_pool(("mul1most", 0), ("prod1", 0), ("gin", 1, 0))
@@ -454,6 +446,7 @@ def tile_gaussian_nn_htanh_v_kernel(
         dve += four("mask", 2) + two("empty1", 2) + [("mul1", 5)] + quant("w2", 1, 1) + dzn(2) + [("mul1", 6), ("mul1", 7)] + dzh(2)
         on_pool(("mul1", 4), ("prod1", 4), ("dzin", 1))
         act += two("abs", 3) + two("empty1", 3) + two("emptyz", 2) + two("emptyg", 0, 1) + two("empty1", 4) + two("empty1", 5)
+
         pe += four("dh", 3) + around(w1(6), w1(7)) + two("turnz", 3) + open_with("mean1", 8) + [("turng", 1, 1)] + close_with("turn1", 8)
         dve += four("mask", 3) + [("mul1rest", 8), ("sort1", 2)] + dzn(3) + quant("g", 0, 1) + quant("w1", 0, 0) + [("weave", 0, 0)] + quant("w1", 1, 0) + dzh(3)
         on_pool(("mul1most", 8), ("prod1", 8), ("dzin", 2))
@@ -467,25 +460,29 @@ def tile_gaussian_nn_htanh_v_kernel(
         on_pool(("mul1", 10), ("prod1", 10), ("dzin", 4))
         pool.append(("mul1most", 11))
         act += [("emptyx", 0, 0, 3)] + two("weave", 1, 1) + two("emptyz", 5) + two("abs", 6) + two("empty1", 10) + two("empty1", 11)
+
         pe += four("dh", 6) + around(w1(12), w1(13)) + two("turnz", 6) + dws("dw", 0, 0, range(4, 8)) + dws("dw", 0, 1, range(4, 8))
         dve += four("mask", 6) + [("mul1rest", 14)] + quant("xq", 1, 1) + quant("xq", 0, 1) + [("mul1high", 15)] + dzn(6) + dws("weigh", 0, 0, range(4, 8)) + dws("weigh", 0, 1, range(4, 8))
         on_pool(("mul1", 13), ("prod1", 13), ("dzin", 5))
         pool += [("mul1most", 14)]
         act += two("weave", 0, 1) + two("empty1", 12) + two("empty1", 13) + two("emptyz", 6) + two("abs", 7)
-        pe += four("dh", 7) + dws("dw", 1, 0, range(4)) + two("turnz", 7) + dws("dw", 1, 0, range(4, 8))
-        dve += four("mask", 7) + dws("weigh", 1, 0, range(4)) + dzh(6) + dzn(7) + dzh(7) + [("add1", 14), ("add1", 15)]
+        pe += four("dh", 7) + dws("dw", 1, 0, range(4)) + two("turnz", 7) + dws("dw", 1, 0, range(4, 8)) + dws("dw", 1, 1, range(1))
+        dve += four("mask", 7) + dws("weigh", 1, 0, range(4)) + dzn(7) + dzh(6) + dzh(7) + [("add1", 14), ("add1", 15)]
         on_pool(("sum", 0, 0), ("total", 0, 0), ("dz", 6))
         pool += [("sum", 0, 1), ("sum", 0, 2), ("mul1low", 15)]
         act += two("emptyz", 7)
         sp += four("store1", 0)[:3]
+        ring = [("dxbank", 1, 0, 0), ("dxbank", 1, 0, 1), ("w1words", 14), ("dxbank", 1, 0, 2), ("w1words", 15), ("dxbank", 1, 0, 3)]
+        for n in range(3, len(ring)):
+            inherits[ring[n]] = ring[n - 3]
         pe += four("dx", 1, 0)[:2] + [("turn1w", 14), ("dx", 1, 0, 2), ("turn1w", 15), ("dx", 1, 0, 3)]
-        dve += dws("weigh", 1, 0, range(4, 8)) + quant("w1", 0, 1) + quant("w1", 1, 1)
+        dve += dws("weigh", 1, 0, range(4, 8)) + dws("weigh", 1, 1, range(1)) + quant("w1", 0, 1) + quant("w1", 1, 1)
         act += four("emptyx", 1, 0)[:2] + [("empty1w", 14), ("emptyx", 1, 0, 2), ("empty1w", 15), ("emptyx", 1, 0, 3)]
-        pe += dws("dw", 1, 1, range(4))
+        pe += dws("dw", 1, 1, range(1, 4))
         for n in range(T):
             pe += [("dx", 0, 1, n)] + dws("dw", 1, 1, range(8)[4 + 2 * n : 6 + 2 * n])
-        pe += four("dx", 1, 1)[:3] + two("dx", 1, 1, 3)
-        dve += dws("weigh", 1, 1, range(6)) + [("sum", 1, 1), ("sum", 1, 2)] + dws("weigh", 1, 1, range(6, 8)) + [("sum", 1, 3)]
+        pe += four("dx", 1, 1)[:3] + two("dx", 1, 1, T - 1)
+        dve += dws("weigh", 1, 1, range(1, 6)) + [("sum", 1, 1), ("sum", 1, 2)] + dws("weigh", 1, 1, range(6, 8)) + [("sum", 1, 3)]
         pool += [("sum", 0, 3), ("sum", 1, 0)]
         inherits["total", 0, 3] = ("prod1", 15)
         act += four("emptyx", 0, 1) + four("emptyx", 1, 1)[:3] + [("emptyx", 1, 1, 3, 0)]
@@ -494,7 +491,6 @@ def tile_gaussian_nn_htanh_v_kernel(
         for n in range(T):
             sp += [("store0", 0, 1, n), ("store1", 1, n)]
         sp += four("store0", 1, 1)[:3] + two("store0", 1, 1, 3)
-
 
         queues = [(nc.tensor, pe), (nc.vector, dve), (nc.scalar, act), (nc.gpsimd, pool), (nc.sync, sp)]
         writers = {}

@@ -21,7 +21,6 @@ BYTES = 2 * (N * X + 2 * X * H + J * X * H + 2 * H * Y + J * H * Y + J * N * Y) 
 P = 128
 T = 4
 K = P * T
-RUN = 8
 
 EDGE = 1.0 + 3.0 / 256.0
 
@@ -101,55 +100,53 @@ def tile_gaussian_nn_htanh_v_kernel(
                 specs[name] = ("bank", shape, F32)
             return names
 
+        def product(engine, out, noise, sig, places):
+            if engine is nc.gpsimd:
+                out, walk = out[:, places], lambda ap: ap.rearrange("p (m t) -> p t m", t=T)[:, places]
+            else:
+                out = out.rearrange("p t (w i) -> p w t i", i=2)[:, :, places]
+                walk = lambda ap: ap.rearrange("p (w i t) -> p w t i", t=T, i=2)[:, :, places]
+            engine.tensor_tensor(out=out, in0=walk(noise), in1=walk(sig), op=ALU.mult)
+
+        shares = {"": (0, T), "most": (0, T - 1), "rest": (T - 1, T), "low": (0, 2), "high": (2, T)}
+
         def w2_load(src, name, a):
-            blocks = 2 if a < 2 else 4
-            load(name + (min(a, 2),), "load", [P, blocks, Y], BF16, src.rearrange("(a b m) y -> a m b y", b=blocks, m=P)[a if a < 2 else 1])
+            rows = src.rearrange("(q p u) y -> q p u y", q=2, u=T)
+            if a < 2:
+                load(name + (a,), "load", [P, 2, Y], BF16, rows[0][:, cols(a, 2), :])
+            else:
+                load(name + (2,), "load", [P, T, Y], BF16, rows[1])
 
         def w2_in(name, a):
-            return tiles[name + (min(a, 2),)][:, cols(max(a - 2, 0), 2), :]
+            return tiles[name + (min(a, 2),)][:, cols(max(a - 2, 0), 2), :].rearrange("p b y -> p (b y)")
 
         def w2_rows(a):
-            q, r = divmod(a, 2)
             for name, src in (("sig2", sig_W2), ("mu2", mu_W2)):
                 w2_load(src, (name,), a)
-            specs["mean2", a] = ("work", [P, T, 2, P], BF16)
-
-            def sort_mean(engine):
-                src = w2_in(("mu2",), a).rearrange("p b (w i t) -> p (b w) t i", t=T, i=4)
-                copy(engine, tiles["mean2", a][:].rearrange("p t b (w i) -> p (b w) t i", i=4), src)
-
-            step(("sort2", a), [("mu2", min(a, 2))], [("mean2", a)], sort_mean)
             for j in range(J):
-                w2_sample(j, a, q, r)
+                w2_sample(j, a, *divmod(a, 2))
 
         def w2_sample(j, a, q, r):
             w2_load(e_W2[j], ("e2", j), a)
-            specs["prod2", j, a] = ("work", [P, T, 2, P], F32)
+            specs["prod2", j, a] = ("work", [P, T, 2 * P], F32)
             specs["w2in", j, q] = ("work", [P, K, T], BF16)
             banks = banks_for(("w2bank", j, a), 2, [P, T, P])
 
-            def multiply(engine):
-                walk = "p b (w i t) -> p (b w) t i"
-                engine.tensor_tensor(
-                    out=tiles["prod2", j, a][:].rearrange("p t b (w i) -> p (b w) t i", i=2),
-                    in0=w2_in(("e2", j), a).rearrange(walk, t=T, i=2),
-                    in1=w2_in(("sig2",), a).rearrange(walk, t=T, i=2),
-                    op=ALU.mult,
-                )
+            def multiply(places, engine):
+                product(engine, tiles["prod2", j, a][:], w2_in(("e2", j), a), w2_in(("sig2",), a), places)
 
-            def turn(source, first, engine):
-                block = w2_in(("mu2",), a).rearrange("p b (w t) -> p t b w", t=T) if source[0] == "mu2" else tiles[source]
-                turn_part(banks, lambda b, t: block[:, t, b, :], source[0] != "prod2", first)
+            def turn(is_mean, first, engine):
+                block = w2_in(("mu2",), a).rearrange("p (m t) -> p t m", t=T) if is_mean else tiles["prod2", j, a][:]
+                turn_part(banks, lambda b, t: block[:, t, cols(b)], is_mean, first)
 
             def empty(b, engine):
-                dst = tiles["w2in", j, q][:].rearrange("p (u b i) t -> p u b i t", u=T, i=RUN)
-                src = tiles[banks[b]][:].rearrange("p t (b u i) -> p u b i t", u=T, i=RUN)
-                copy(engine, dst[:, :, cols(2 * r + b, 4), :, :], src)
+                copy(engine, tiles["w2in", j, q][:, cols(2 * r + b), :], tiles[banks[b]][:].rearrange("p t m -> p m t"))
 
-            step(("mul2", j, a), [("e2", j, min(a, 2)), ("sig2", min(a, 2))], [("prod2", j, a)], multiply)
+            for name, places in shares.items():
+                step(("mul2" + name, j, a), [("e2", j, min(a, 2)), ("sig2", min(a, 2))], [("prod2", j, a)], partial(multiply, slice(*places)))
             for first in (False, True):
-                for name, source in (("turn2", ("prod2", j, a)), ("mean2", ("mean2", a)), ("raw2", ("mu2", min(a, 2)))):
-                    step((name, j, a, first), [source], banks, partial(turn, source, first))
+                step(("turn2", j, a, first), [("prod2", j, a)], banks, partial(turn, False, first))
+                step(("mean2", j, a, first), [("mu2", min(a, 2))], banks, partial(turn, True, first))
             for b in range(2):
                 step(("empty2", j, a, b), [banks[b]], [("w2in", j, q)], partial(empty, b))
             quantize(("w2", j, q), E4M3, ("w2in", j, q))
@@ -180,66 +177,50 @@ def tile_gaussian_nn_htanh_v_kernel(
             load(("x", g, xh), "load", [P, T, K], BF16, x.rearrange("(g p t) w -> g p t w", g=2, t=T)[g][:, :, cols(xh, K)])
             specs["xin", g, xh] = ("work", [P, K, T], BF16)
 
-            def interleave(part, engine):
-                src = tiles["x", g, xh][:, :, part].rearrange("p t (c i) -> p c t i", i=4)
-                copy(engine, tiles["xin", g, xh][:, part, :].rearrange("p (c i) t -> p c t i", i=4), src)
+            def interleave(n, engine):
+                src = tiles["x", g, xh][:, :, cols(n, 2 * P)].rearrange("p t (c i r) -> p c t i r", i=2, r=2)
+                copy(engine, tiles["xin", g, xh][:, cols(n, 2 * P), :].rearrange("p (r c i) t -> p c t i r", i=2, r=2), src)
 
             for n in range(2):
-                step(("weave", g, xh, n), [("x", g, xh)], [("xin", g, xh)], partial(interleave, cols(n, K // 2)))
-            step(("weave", g, xh), [("x", g, xh)], [("xin", g, xh)], partial(interleave, cols(0, K)))
+                step(("weave", g, xh, n), [("x", g, xh)], [("xin", g, xh)], partial(interleave, n))
             quantize(("xq", g, xh), E4M3, ("xin", g, xh))
 
         def w1_pair(a):
-            for name, src in (("sig1", sig_W1), ("mu1", mu_W1)):
-                load((name, a), "load", [P, 2, H], BF16, src.rearrange("(a r m) h -> a m r h", r=2, m=P)[a])
-            specs["mean1", a] = ("work", [P, 2, T, 32, RUN], BF16)
-
-            def sort_mean(engine):
-                copy(engine, tiles["mean1", a][:], tiles["mu1", a][:].rearrange("p r (b u i) -> p r u b i", u=T, i=RUN))
-
-            step(("sort1", a), [("mu1", a)], [("mean1", a)], sort_mean)
+            for name, src in ((("sig1",), sig_W1), (("mu1",), mu_W1), (("e1", 0), e_W1[0]), (("e1", 1), e_W1[1])):
+                load(name + (a,), "load", [P, 2, H], BF16, src.rearrange("(a m r) h -> a m r h", r=2, m=P)[a])
             for i in (2 * a, 2 * a + 1):
-                load(("e1", i), "load", [P, J, H], BF16, e_W1[:, cols(i), :].rearrange("j m h -> m j h"))
                 for j in range(J):
                     w1_block(i, j)
 
         def w1_block(i, j):
             a, r = divmod(i, 2)
             xh, c = divmod(i, 4)
-            n = J * i + j
-            specs["prod1", n] = ("work", [P, T, 32, RUN], F32)
-            specs["sum1", n] = ("work", [P, 2, 2 * P, 2], BF16)
+            n = 4 * a + 2 * j + r
+            specs["prod1", n] = ("work", [P, T, 2 * P], F32)
+            specs["flat1", n] = ("work", [P, H], F32)
+            specs["sum1", n] = ("work", [P, H], BF16)
             specs["w1in", j, xh] = ("w1in", [P, 2 * K, T], BF16)
             banks = banks_for(("w1bank", n), 2, [P, T, P])
             specs["w1words", n] = ("bank", [P, 2, 2, P], F32)
 
             def multiply(places, engine):
-                sort = "p (b u i) -> p u b i"
-                engine.tensor_tensor(
-                    out=tiles["prod1", n][:, places],
-                    in0=tiles["e1", i][:, j, :].rearrange(sort, u=T, i=RUN)[:, places],
-                    in1=tiles["sig1", a][:, r, :].rearrange(sort, u=T, i=RUN)[:, places],
-                    op=ALU.mult,
-                )
+                product(engine, tiles["prod1", n][:], tiles["e1", j, a][:, r, :], tiles["sig1", a][:, r, :], places)
 
             def turn(is_mean, first, engine):
-                block = (tiles["mean1", a][:, r] if is_mean else tiles["prod1", n][:]).rearrange("p u (q b) i -> p u q (b i)", q=2)
-                turn_part(banks, lambda q, u: block[:, u, q, :], is_mean, first)
+                block = tiles["mu1", a][:, r, :].rearrange("p (m u) -> p u m", u=T) if is_mean else tiles["prod1", n][:]
+                turn_part(banks, lambda q, u: block[:, u, cols(q)], is_mean, first)
 
             def empty(q, engine):
                 copy(engine, tiles["w1in", j, xh][:, cols(T * q + c), :], tiles[banks[q]][:].rearrange("p u m -> p m u"))
 
+            def multiply_flat(part, engine):
+                engine.tensor_tensor(out=tiles["flat1", n][:, part], in0=tiles["e1", j, a][:, r, part], in1=tiles["sig1", a][:, r, part], op=ALU.mult)
+
             def add_mean(engine):
-                pair = "p (s e) b i -> p s (b i) e"
-                engine.tensor_tensor(
-                    out=tiles["sum1", n][:],
-                    in0=tiles["prod1", n][:].rearrange(pair, e=2),
-                    in1=tiles["mean1", a][:, r].rearrange(pair, e=2),
-                    op=ALU.add,
-                )
+                engine.tensor_tensor(out=tiles["sum1", n][:], in0=tiles["flat1", n][:], in1=tiles["mu1", a][:, r, :], op=ALU.add)
 
             def turn_words(engine):
-                words = tiles["sum1", n][:].rearrange("p s m e -> p (s m e)").bitcast(F32).rearrange("p (s q m) -> p q s m", s=2, q=2)
+                words = tiles["sum1", n][:].bitcast(F32).rearrange("p (q m s) -> p q s m", s=2, q=2)
                 for q in range(2):
                     for s in range(2):
                         engine.transpose(tiles["w1words", n][:, q, s, :], words[:, q, s, :], ident_f[:])
@@ -248,15 +229,15 @@ def tile_gaussian_nn_htanh_v_kernel(
                 dst = tiles["w1in", j, xh][:].rearrange("p c t -> p (c t)").bitcast(F32).rearrange("p (q c m s) -> p q c m s", q=2, m=P, s=2)
                 copy(engine, dst[:, :, c], tiles["w1words", n][:].rearrange("p q s m -> p q m s"))
 
-            shares = {"mul1": (0, T), "mul1most": (0, T - 1), "mul1rest": (T - 1, T), "mul1low": (0, 2), "mul1high": (2, T)}
             for name, places in shares.items():
-                step((name, n), [("e1", i), ("sig1", a)], [("prod1", n)], partial(multiply, slice(*places)))
+                step(("mul1" + name, n), [("e1", j, a), ("sig1", a)], [("prod1", n)], partial(multiply, slice(*places)))
+                step(("flat" + name, n), [("e1", j, a), ("sig1", a)], [("flat1", n)], partial(multiply_flat, slice(2 * P * places[0], 2 * P * places[1])))
             for first in (False, True):
                 step(("turn1", n, first), [("prod1", n)], banks, partial(turn, False, first))
-                step(("mean1", n, first), [("mean1", a)], banks, partial(turn, True, first))
+                step(("mean1", n, first), [("mu1", a)], banks, partial(turn, True, first))
             for q in range(2):
                 step(("empty1", n, q), [banks[q]], [("w1in", j, xh)], partial(empty, q))
-            step(("add1", n), [("prod1", n), ("mean1", a)], [("sum1", n)], add_mean)
+            step(("add1", n), [("flat1", n), ("mu1", a)], [("sum1", n)], add_mean)
             step(("turn1w", n), [("sum1", n)], [("w1words", n)], turn_words)
             step(("empty1w", n), [("w1words", n)], [("w1in", j, xh)], empty_words)
             quantize(("w1", j, xh), E4M3, ("w1in", j, xh), kind="wide")
@@ -269,9 +250,9 @@ def tile_gaussian_nn_htanh_v_kernel(
             dh = banks_for(("dhbank", k), T, [P, T, P])
             turned = banks_for(("dzbank", k), 2, [P, T, P])
 
-            def absolute(n, engine):
-                dst = tiles["abs", k][:, cols(n, K // 2), :].rearrange("p (c i) t -> p c t i", i=4)
-                src = tiles["z", k][:, :, cols(n, K // 2)].rearrange("p t (c i) -> p c t i", i=4)
+            def absolute(part, engine):
+                dst = tiles["abs", k][:, part, :].rearrange("p (c i) t -> p c t i", i=4)
+                src = tiles["z", k][:, :, part].rearrange("p t (c i) -> p c t i", i=4)
                 engine.activation(out=dst, in_=src, func=ACT.Abs, scale=EDGE)
 
             def multiply(u, engine):
@@ -279,10 +260,9 @@ def tile_gaussian_nn_htanh_v_kernel(
                     mx(tiles[dh[u]][:, t, :], ("g", j, g), cols(t), E5M2, ("w2", j, q), cols(u), E4M3, True, True)
 
             def mask(u, engine):
-                dz = tiles["dz", k][:].rearrange("p (u b i) t -> p u b i t", u=T, i=RUN)
-                size = tiles["abs", k][:].rearrange("p (b u i) t -> p u b i t", u=T, i=RUN)
-                bank = tiles[dh[u]][:].rearrange("p t (b i) -> p b i t", i=RUN)
-                engine.scalar_tensor_tensor(out=dz[:, u], in0=size[:, u], scalar=EDGE, in1=bank, op0=ALU.is_lt, op1=ALU.mult)
+                size = tiles["abs", k][:].rearrange("p (m u) t -> p u m t", u=T)
+                bank = tiles[dh[u]][:].rearrange("p t m -> p m t")
+                engine.scalar_tensor_tensor(out=tiles["dz", k][:, cols(u), :], in0=size[:, u], scalar=EDGE, in1=bank, op0=ALU.is_lt, op1=ALU.mult)
 
             def turn(s, engine):
                 words = tiles["dz", k][:].rearrange("p c t -> p (c t)").bitcast(F32).rearrange("p (u m s) -> p s u m", u=T, s=2)
@@ -293,8 +273,9 @@ def tile_gaussian_nn_htanh_v_kernel(
                 src = tiles[turned[s]][:].bitcast(BF16).rearrange("p u (m e) -> p e m u", e=2)
                 copy(engine, tiles["dzin", k][:, cols(s, K // 2), :].rearrange("p (e m) u -> p e m u", e=2), src)
 
+            step(("abs", k), [("z", k)], [("abs", k)], partial(absolute, cols(0, K)))
             for n in range(2):
-                step(("abs", k, n), [("z", k)], [("abs", k)], partial(absolute, n))
+                step(("abs", k, n), [("z", k)], [("abs", k)], partial(absolute, cols(n, K // 2)))
                 step(("turnz", k, n), [("dz", k)], [turned[n]], partial(turn, n))
                 step(("emptyz", k, n), [turned[n]], [("dzin", k)], partial(empty, n))
             for u in range(T):
@@ -316,12 +297,15 @@ def tile_gaussian_nn_htanh_v_kernel(
                     columns = cols(pieces * q + piece, width)
                     mx(tiles[bank][:], ("dzh", j, q, g), cols(t), E5M2, ("w1", j, xh), columns, E4M3, (q, j) == passes[0], (q, j) == passes[-1])
 
+            def empty(engine):
+                copy(engine, tiles[out][:].rearrange("p (n m r) -> p n m r", m=P, r=2), tiles[bank][:].rearrange("p (n r m) -> p n m r", m=P, r=2))
+
             def store(engine):
                 view = out_0.rearrange("(g p t) w -> g p t w", g=2, t=T)[g]
                 engine.dma_start(out=view[:, t, cols(pieces * xh + piece, width)], in_=tiles[out][:])
 
             step(("dx",) + key, [("dzh", j, q, g) for q, j in passes] + [("w1", j, xh) for j in range(J)], [bank], multiply)
-            step(("emptyx",) + key, [bank], [out], lambda engine: copy(engine, tiles[out][:], tiles[bank][:]))
+            step(("emptyx",) + key, [bank], [out], empty)
             step(("store0",) + key, [out], [], store)
 
         def dw(q, i, j):
@@ -329,7 +313,6 @@ def tile_gaussian_nn_htanh_v_kernel(
             part = ("part", q, i // 2, j)
             specs[bank] = ("bank", [P, K], F32)
             specs[part] = ("work", [P, 2, K], F32)
-            natural = "p (b u i) -> p b u i"
 
             def multiply(engine):
                 for g in range(2):
@@ -337,14 +320,14 @@ def tile_gaussian_nn_htanh_v_kernel(
 
             def weigh(engine):
                 engine.tensor_tensor(
-                    out=tiles[part][:, i % 2, :].rearrange(natural, u=T, i=RUN),
-                    in0=tiles["e1", i][:, j, cols(q, K)].rearrange(natural, u=T, i=RUN),
-                    in1=tiles[bank][:].rearrange("p (u b i) -> p b u i", u=T, i=RUN),
+                    out=tiles[part][:, i % 2, :].rearrange("p (m u) -> p m u", u=T),
+                    in0=tiles["e1", j, i // 2][:, i % 2, cols(q, K)].rearrange("p (m u) -> p m u", u=T),
+                    in1=tiles[bank][:].rearrange("p (u m) -> p m u", u=T),
                     op=ALU.mult,
                 )
 
             step(("dw", q, i, j), [("xq", g, i // 4) for g in range(2)] + [("dzn", j, q, g) for g in range(2)], [bank], multiply)
-            step(("weigh", q, i, j), [("e1", i), bank], [part], weigh)
+            step(("weigh", q, i, j), [("e1", j, i // 2), bank], [part], weigh)
 
         def dw_sum(q, a):
             first, second, total = ("part", q, a, 0), ("part", q, a, 1), ("total", q, a)
@@ -354,7 +337,7 @@ def tile_gaussian_nn_htanh_v_kernel(
                 engine.tensor_tensor(out=tiles[total][:], in0=tiles[first][:], in1=tiles[second][:], op=ALU.add)
 
             def store(engine):
-                view = out_1.rearrange("(a r m) h -> a m r h", r=2, m=P)[a][:, :, cols(q, K)]
+                view = out_1.rearrange("(a m r) h -> a m r h", r=2, m=P)[a][:, :, cols(q, K)]
                 engine.dma_start(out=view, in_=tiles[total][:])
 
             step(("sum", q, a), [first, second], [total], add)
@@ -410,8 +393,8 @@ def tile_gaussian_nn_htanh_v_kernel(
         def close_with(name, *key):
             return [(name,) + key + (False,)]
 
-        def w2(j, a, mean):
-            return (("turn2", j, a), (mean, j, a))
+        def w2(j, a):
+            return (("turn2", j, a), ("mean2", j, a))
 
         def w1(n):
             return (("turn1", n), ("mean1", n))
@@ -427,19 +410,19 @@ def tile_gaussian_nn_htanh_v_kernel(
 
         sp += loads(("sig2", 0), ("e2", 0, 0), ("mu2", 0), ("sig2", 1), ("e2", 0, 1), ("mu2", 1), ("grad", 0, 0), ("e2", 1, 0), ("e2", 1, 1), ("z", 0))
         sp += loads(("grad", 1, 0), ("sig2", 2), ("e2", 0, 2), ("mu2", 2), ("z", 1), ("e2", 1, 2))
-        sp += loads(("sig1", 0), ("e1", 0), ("mu1", 0), ("z", 2), ("e1", 1), ("sig1", 1), ("e1", 2), ("mu1", 1), ("z", 3), ("grad", 0, 1), ("e1", 3))
-        sp += loads(("sig1", 2), ("e1", 4), ("z", 4), ("mu1", 2), ("grad", 1, 1), ("x", 0, 0), ("z", 5), ("x", 1, 0), ("mu1", 3), ("e1", 5), ("x", 1, 1))
-        sp += loads(("z", 6), ("sig1", 3), ("e1", 6), ("x", 0, 1), ("e1", 7))
+        sp += loads(("sig1", 0), ("e1", 0, 0), ("mu1", 0), ("z", 2), ("e1", 1, 0), ("sig1", 1), ("e1", 0, 1), ("mu1", 1), ("z", 3), ("grad", 0, 1), ("e1", 1, 1))
+        sp += loads(("sig1", 2), ("e1", 0, 2), ("z", 4), ("mu1", 2), ("grad", 1, 1), ("x", 0, 0), ("z", 5), ("x", 1, 0), ("mu1", 3), ("e1", 1, 2), ("x", 1, 1))
+        sp += loads(("z", 6), ("sig1", 3), ("e1", 0, 3), ("x", 0, 1), ("e1", 1, 3))
         sp += four("store0", 0, 0) + loads(("z", 7))
-        pe += products_first(w2(0, 0, "mean2")) + means_first(w2(0, 1, "mean2")) + [("turng", 0, 0)] + around(w2(1, 0, "mean2"), w2(1, 1, "mean2"))
+        pe += products_first(w2(0, 0)) + means_first(w2(0, 1)) + [("turng", 0, 0)] + around(w2(1, 0), w2(1, 1))
         dve += [("mul2", 0, 0), ("mul2", 0, 1), ("mul2", 1, 0), ("mul2", 1, 1)] + two("emptyg", 0, 0) + quant("w2", 0, 0) + quant("g", 0, 0) + [("empty2", 1, 0, 0)]
-        act += [("sort2", 0), ("sort2", 1)] + two("empty2", 0, 0) + two("empty2", 0, 1) + two("abs", 0) + [("empty2", 1, 0, 1)] + two("empty2", 1, 1)
-        pe += four("dh", 0) + [("turng", 1, 0)] + two("turnz", 0) + four("dh", 1) + products_first(w2(0, 2, "raw2")) + means_first(w2(0, 3, "raw2"))
+        act += two("empty2", 0, 0) + two("empty2", 0, 1) + two("abs", 0) + [("empty2", 1, 0, 1)] + two("empty2", 1, 1)
+        pe += four("dh", 0) + [("turng", 1, 0)] + two("turnz", 0) + four("dh", 1) + products_first(w2(0, 2)) + means_first(w2(0, 3))
         dve += four("mask", 0) + quant("w2", 1, 0) + quant("g", 1, 0) + [("mul2", 0, 2)] + dzn(0) + [("mul2", 0, 3), ("mul2", 1, 2)]
         act += two("emptyg", 1, 0) + two("emptyz", 0) + two("abs", 1) + two("empty2", 0, 2) + two("empty2", 0, 3)
 
-        pe += products_first(w2(1, 2, "raw2")) + two("turnz", 1) + means_first(w2(1, 3, "raw2")) + around(w1(0), w1(1))
-        dve += four("mask", 1) + [("mul1rest", 0), ("mul2", 1, 3), ("sort1", 0)] + dzn(1) + [("mul1", 1)] + quant("w2", 0, 1) + dzh(0) + [("mul1", 2), ("mul1", 3), ("sort1", 1)] + dzh(1)
+        pe += products_first(w2(1, 2)) + two("turnz", 1) + means_first(w2(1, 3)) + around(w1(0), w1(1))
+        dve += four("mask", 1) + [("mul1rest", 0), ("mul2", 1, 3)] + dzn(1) + [("mul1", 1)] + quant("w2", 0, 1) + dzh(0) + [("mul1", 2), ("mul1", 3)] + dzh(1)
         on_pool(("mul1most", 0), ("prod1", 0), ("gin", 1, 0))
         act += two("empty2", 1, 2) + two("abs", 2) + two("emptyz", 1) + two("empty2", 1, 3) + two("empty1", 0) + two("empty1", 1)
         pe += four("dh", 2) + around(w1(2), w1(3)) + two("turnz", 2) + open_with("mean1", 4) + [("turng", 0, 1)] + open_with("mean1", 5) + close_with("turn1", 4) + close_with("turn1", 5)
@@ -448,11 +431,11 @@ def tile_gaussian_nn_htanh_v_kernel(
         act += two("abs", 3) + two("empty1", 3) + two("emptyz", 2) + two("emptyg", 0, 1) + two("empty1", 4) + two("empty1", 5)
 
         pe += four("dh", 3) + around(w1(6), w1(7)) + two("turnz", 3) + open_with("mean1", 8) + [("turng", 1, 1)] + close_with("turn1", 8)
-        dve += four("mask", 3) + [("mul1rest", 8), ("sort1", 2)] + dzn(3) + quant("g", 0, 1) + quant("w1", 0, 0) + [("weave", 0, 0)] + quant("w1", 1, 0) + dzh(3)
+        dve += four("mask", 3) + [("mul1rest", 8)] + dzn(3) + quant("g", 0, 1) + quant("w1", 0, 0) + two("weave", 0, 0) + quant("w1", 1, 0) + dzh(3)
         on_pool(("mul1most", 8), ("prod1", 8), ("dzin", 2))
         act += two("abs", 4) + two("empty1", 6) + two("empty1", 7) + two("emptyz", 3) + two("emptyg", 1, 1)
         pe += four("dh", 4) + four("dx", 0, 0)[:3] + two("turnz", 4) + means_first(w1(9)) + [("dx", 0, 0, 3)]
-        dve += four("mask", 4) + [("mul1rest", 9)] + quant("xq", 0, 0) + dzn(4) + quant("g", 1, 1) + [("weave", 1, 0), ("sort1", 3)] + quant("xq", 1, 0) + dzh(4)
+        dve += four("mask", 4) + [("mul1rest", 9)] + quant("xq", 0, 0) + dzn(4) + quant("g", 1, 1) + two("weave", 1, 0) + quant("xq", 1, 0) + dzh(4)
         on_pool(("mul1most", 9), ("prod1", 9), ("dzin", 3))
         act += two("empty1", 8) + two("abs", 5) + four("emptyx", 0, 0)[:3] + two("emptyz", 4) + two("empty1", 9)
         pe += four("dh", 5) + dws("dw", 0, 0, range(4)) + two("turnz", 5) + around(w1(10), w1(11)) + dws("dw", 0, 1, range(4))
@@ -462,14 +445,14 @@ def tile_gaussian_nn_htanh_v_kernel(
         act += [("emptyx", 0, 0, 3)] + two("weave", 1, 1) + two("emptyz", 5) + two("abs", 6) + two("empty1", 10) + two("empty1", 11)
 
         pe += four("dh", 6) + around(w1(12), w1(13)) + two("turnz", 6) + dws("dw", 0, 0, range(4, 8)) + dws("dw", 0, 1, range(4, 8))
-        dve += four("mask", 6) + [("mul1rest", 14)] + quant("xq", 1, 1) + quant("xq", 0, 1) + [("mul1high", 15)] + dzn(6) + dws("weigh", 0, 0, range(4, 8)) + dws("weigh", 0, 1, range(4, 8))
+        dve += four("mask", 6) + [("flatrest", 14)] + quant("xq", 1, 1) + quant("xq", 0, 1) + [("flathigh", 15)] + dzn(6) + dws("weigh", 0, 0, range(4, 8)) + dws("weigh", 0, 1, range(4, 8))
         on_pool(("mul1", 13), ("prod1", 13), ("dzin", 5))
-        pool += [("mul1most", 14)]
+        pool += [("flatmost", 14)]
         act += two("weave", 0, 1) + two("empty1", 12) + two("empty1", 13) + two("emptyz", 6) + two("abs", 7)
         pe += four("dh", 7) + dws("dw", 1, 0, range(4)) + two("turnz", 7) + dws("dw", 1, 0, range(4, 8)) + dws("dw", 1, 1, range(1))
         dve += four("mask", 7) + dws("weigh", 1, 0, range(4)) + dzn(7) + dzh(6) + dzh(7) + [("add1", 14), ("add1", 15)]
         on_pool(("sum", 0, 0), ("total", 0, 0), ("dz", 6))
-        pool += [("sum", 0, 1), ("sum", 0, 2), ("mul1low", 15)]
+        pool += [("sum", 0, 1), ("sum", 0, 2), ("flatlow", 15)]
         act += two("emptyz", 7)
         sp += four("store1", 0)[:3]
         ring = [("dxbank", 1, 0, 0), ("dxbank", 1, 0, 1), ("w1words", 14), ("dxbank", 1, 0, 2), ("w1words", 15), ("dxbank", 1, 0, 3)]
@@ -484,7 +467,7 @@ def tile_gaussian_nn_htanh_v_kernel(
         pe += four("dx", 1, 1)[:3] + two("dx", 1, 1, T - 1)
         dve += dws("weigh", 1, 1, range(1, 6)) + [("sum", 1, 1), ("sum", 1, 2)] + dws("weigh", 1, 1, range(6, 8)) + [("sum", 1, 3)]
         pool += [("sum", 0, 3), ("sum", 1, 0)]
-        inherits["total", 0, 3] = ("prod1", 15)
+        inherits["total", 0, 3] = ("flat1", 15)
         act += four("emptyx", 0, 1) + four("emptyx", 1, 1)[:3] + [("emptyx", 1, 1, 3, 0)]
         dve.append(("emptyx", 1, 1, 3, 1))
         sp += four("store0", 1, 0)[:2] + [("store1", 0, 3)] + four("store0", 1, 0)[2:]

@@ -108,6 +108,12 @@ def tile_gaussian_nn_htanh_v_kernel(
                 walk = lambda ap: ap.rearrange("p (w i t) -> p w t i", t=T, i=2)[:, :, places]
             engine.tensor_tensor(out=out, in0=walk(noise), in1=walk(sig), op=ALU.mult)
 
+        def sort_words(engine, out, mean):
+            copy(engine, out, mean.bitcast(F32).rearrange("p (m s) -> p s m", s=2))
+
+        def sorted_place(words, t):
+            return words[:, t // 2, :].bitcast(BF16).rearrange("p (m e) -> p e m", e=2)[:, t % 2, :]
+
         shares = {"": (0, T), "most": (0, T - 1), "rest": (T - 1, T), "low": (0, 2), "high": (2, T)}
 
         def w2_load(src, name, a):
@@ -123,6 +129,8 @@ def tile_gaussian_nn_htanh_v_kernel(
         def w2_rows(a):
             for name, src in (("sig2", sig_W2), ("mu2", mu_W2)):
                 w2_load(src, (name,), a)
+            specs["mean2", a] = ("work", [P, 2, 2 * P], F32)
+            step(("sort2", a), [("mu2", min(a, 2))], [("mean2", a)], lambda engine: sort_words(engine, tiles["mean2", a][:], w2_in(("mu2",), a)))
             for j in range(J):
                 w2_sample(j, a, *divmod(a, 2))
 
@@ -139,6 +147,9 @@ def tile_gaussian_nn_htanh_v_kernel(
                 block = w2_in(("mu2",), a).rearrange("p (m t) -> p t m", t=T) if is_mean else tiles["prod2", j, a][:]
                 turn_part(banks, lambda b, t: block[:, t, cols(b)], is_mean, first)
 
+            def turn_sorted(first, engine):
+                turn_part(banks, lambda b, t: sorted_place(tiles["mean2", a][:], t)[:, cols(b)], True, first)
+
             def empty(b, engine):
                 copy(engine, tiles["w2in", j, q][:, cols(2 * r + b), :], tiles[banks[b]][:].rearrange("p t m -> p m t"))
 
@@ -146,7 +157,8 @@ def tile_gaussian_nn_htanh_v_kernel(
                 step(("mul2" + name, j, a), [("e2", j, min(a, 2)), ("sig2", min(a, 2))], [("prod2", j, a)], partial(multiply, slice(*places)))
             for first in (False, True):
                 step(("turn2", j, a, first), [("prod2", j, a)], banks, partial(turn, False, first))
-                step(("mean2", j, a, first), [("mu2", min(a, 2))], banks, partial(turn, True, first))
+                step(("raw2", j, a, first), [("mu2", min(a, 2))], banks, partial(turn, True, first))
+                step(("mean2", j, a, first), [("mean2", a)], banks, partial(turn_sorted, first))
             for b in range(2):
                 step(("empty2", j, a, b), [banks[b]], [("w2in", j, q)], partial(empty, b))
             quantize(("w2", j, q), E4M3, ("w2in", j, q))
@@ -188,6 +200,8 @@ def tile_gaussian_nn_htanh_v_kernel(
         def w1_pair(a):
             for name, src in ((("sig1",), sig_W1), (("mu1",), mu_W1), (("e1", 0), e_W1[0]), (("e1", 1), e_W1[1])):
                 load(name + (a,), "load", [P, 2, H], BF16, src.rearrange("(a m r) h -> a m r h", r=2, m=P)[a])
+            specs["mean1", a] = ("work", [P, 2, K], F32)
+            step(("sort1", a), [("mu1", a)], [("mean1", a)], lambda engine: sort_words(engine, tiles["mean1", a][:], tiles["mu1", a][:].rearrange("p r h -> p (r h)")))
             for i in (2 * a, 2 * a + 1):
                 for j in range(J):
                     w1_block(i, j)
@@ -210,6 +224,9 @@ def tile_gaussian_nn_htanh_v_kernel(
                 block = tiles["mu1", a][:, r, :].rearrange("p (m u) -> p u m", u=T) if is_mean else tiles["prod1", n][:]
                 turn_part(banks, lambda q, u: block[:, u, cols(q)], is_mean, first)
 
+            def turn_sorted(first, engine):
+                turn_part(banks, lambda q, u: sorted_place(tiles["mean1", a][:], u)[:, cols(2 * r + q)], True, first)
+
             def empty(q, engine):
                 copy(engine, tiles["w1in", j, xh][:, cols(T * q + c), :], tiles[banks[q]][:].rearrange("p u m -> p m u"))
 
@@ -218,6 +235,24 @@ def tile_gaussian_nn_htanh_v_kernel(
 
             def add_mean(engine):
                 engine.tensor_tensor(out=tiles["sum1", n][:], in0=tiles["flat1", n][:], in1=tiles["mu1", a][:, r, :], op=ALU.add)
+
+            def add_sorted(engine):
+                walk = "p (m s e) -> p m s e"
+                engine.tensor_tensor(
+                    out=tiles["sum1", n][:].rearrange("p (s m e) -> p m s e", s=2, e=2),
+                    in0=tiles["flat1", n][:].rearrange(walk, s=2, e=2),
+                    in1=tiles["mu1", a][:, r, :].rearrange(walk, s=2, e=2),
+                    op=ALU.add,
+                )
+
+            def turn_sorted_words(engine):
+                words = tiles["sum1", n][:].bitcast(F32).rearrange("p (s q m) -> p q s m", s=2, q=2)
+                for q in range(2):
+                    for s in range(2):
+                        engine.transpose(tiles["w1words", n][:, q, s, :], words[:, q, s, :], ident_f[:])
+
+            step(("add1s", n), [("flat1", n), ("mu1", a)], [("sum1", n)], add_sorted)
+            step(("turn1s", n), [("sum1", n)], [("w1words", n)], turn_sorted_words)
 
             def turn_words(engine):
                 words = tiles["sum1", n][:].bitcast(F32).rearrange("p (q m s) -> p q s m", s=2, q=2)
@@ -234,7 +269,8 @@ def tile_gaussian_nn_htanh_v_kernel(
                 step(("flat" + name, n), [("e1", j, a), ("sig1", a)], [("flat1", n)], partial(multiply_flat, slice(2 * P * places[0], 2 * P * places[1])))
             for first in (False, True):
                 step(("turn1", n, first), [("prod1", n)], banks, partial(turn, False, first))
-                step(("mean1", n, first), [("mu1", a)], banks, partial(turn, True, first))
+                step(("raw1", n, first), [("mu1", a)], banks, partial(turn, True, first))
+                step(("mean1", n, first), [("mean1", a)], banks, partial(turn_sorted, first))
             for q in range(2):
                 step(("empty1", n, q), [banks[q]], [("w1in", j, xh)], partial(empty, q))
             step(("add1", n), [("flat1", n), ("mu1", a)], [("sum1", n)], add_mean)
@@ -273,6 +309,25 @@ def tile_gaussian_nn_htanh_v_kernel(
                 src = tiles[turned[s]][:].bitcast(BF16).rearrange("p u (m e) -> p e m u", e=2)
                 copy(engine, tiles["dzin", k][:, cols(s, K // 2), :].rearrange("p (e m) u -> p e m u", e=2), src)
 
+            specs["dzs", k] = ("work", [P, 2, K], F32)
+
+            def turn_sorted(s, engine):
+                for u in range(T):
+                    engine.transpose(tiles[turned[s]][:, u, :], tiles["dzs", k][:, s, cols(u)], ident_f[:])
+
+            step(("sortz", k), [("dz", k)], [("dzs", k)], lambda engine: sort_words(engine, tiles["dzs", k][:], tiles["dz", k][:].rearrange("p c t -> p (c t)")))
+            for n in range(2):
+                step(("turnzs", k, n), [("dzs", k)], [turned[n]], partial(turn_sorted, n))
+            zview = z1[j].rearrange("(g p t) h -> g p t h", g=2, t=T)[g]
+
+            def absolute_half(n, engine):
+                dst = tiles["abs", k][:, cols(n, K // 2), :].rearrange("p (c i) t -> p c t i", i=4)
+                src = tiles["zhalf", k, n][:].rearrange("p t (c i) -> p c t i", i=4)
+                engine.activation(out=dst, in_=src, func=ACT.Abs, scale=EDGE)
+
+            for n in range(2):
+                load(("zhalf", k, n), "load", [P, T, K // 2], F32, zview[:, :, cols(2 * q + n, K // 2)])
+                step(("abshalf", k, n), [("zhalf", k, n)], [("abs", k)], partial(absolute_half, n))
             step(("abs", k), [("z", k)], [("abs", k)], partial(absolute, cols(0, K)))
             for n in range(2):
                 step(("abs", k, n), [("z", k)], [("abs", k)], partial(absolute, cols(n, K // 2)))
@@ -292,8 +347,8 @@ def tile_gaussian_nn_htanh_v_kernel(
             specs[out] = ("work", [P, width], F32)
             passes = [(q, j) for q in range(2) for j in range(J)]
 
-            def multiply(engine):
-                for q, j in passes:
+            def multiply(some, engine):
+                for q, j in some:
                     columns = cols(pieces * q + piece, width)
                     mx(tiles[bank][:], ("dzh", j, q, g), cols(t), E5M2, ("w1", j, xh), columns, E4M3, (q, j) == passes[0], (q, j) == passes[-1])
 
@@ -304,7 +359,8 @@ def tile_gaussian_nn_htanh_v_kernel(
                 view = out_0.rearrange("(g p t) w -> g p t w", g=2, t=T)[g]
                 engine.dma_start(out=view[:, t, cols(pieces * xh + piece, width)], in_=tiles[out][:])
 
-            step(("dx",) + key, [("dzh", j, q, g) for q, j in passes] + [("w1", j, xh) for j in range(J)], [bank], multiply)
+            for name, some in (("dx", passes), ("dxopen", passes[:-1]), ("dxclose", passes[-1:])):
+                step((name,) + key, [("dzh", j, q, g) for q, j in some] + [("w1", j, xh) for j in sorted(set(j for q, j in some))], [bank], partial(multiply, some))
             step(("emptyx",) + key, [bank], [out], empty)
             step(("store0",) + key, [out], [], store)
 
@@ -393,11 +449,11 @@ def tile_gaussian_nn_htanh_v_kernel(
         def close_with(name, *key):
             return [(name,) + key + (False,)]
 
-        def w2(j, a):
-            return (("turn2", j, a), ("mean2", j, a))
+        def w2(j, a, mean):
+            return (("turn2", j, a), (mean, j, a))
 
-        def w1(n):
-            return (("turn1", n), ("mean1", n))
+        def w1(n, mean="mean1"):
+            return (("turn1", n), (mean, n))
 
         def products_first(*jobs):
             return [job[0] + (True,) for job in jobs] + [job[1] + (False,) for job in jobs]
@@ -414,15 +470,15 @@ def tile_gaussian_nn_htanh_v_kernel(
         sp += loads(("sig1", 2), ("e1", 0, 2), ("z", 4), ("mu1", 2), ("grad", 1, 1), ("x", 0, 0), ("z", 5), ("x", 1, 0), ("mu1", 3), ("e1", 1, 2), ("x", 1, 1))
         sp += loads(("z", 6), ("sig1", 3), ("e1", 0, 3), ("x", 0, 1), ("e1", 1, 3))
         sp += four("store0", 0, 0) + loads(("z", 7))
-        pe += products_first(w2(0, 0)) + means_first(w2(0, 1)) + [("turng", 0, 0)] + around(w2(1, 0), w2(1, 1))
+        pe += products_first(w2(0, 0, "mean2")) + means_first(w2(0, 1, "mean2")) + [("turng", 0, 0)] + around(w2(1, 0, "mean2"), w2(1, 1, "mean2"))
         dve += [("mul2", 0, 0), ("mul2", 0, 1), ("mul2", 1, 0), ("mul2", 1, 1)] + two("emptyg", 0, 0) + quant("w2", 0, 0) + quant("g", 0, 0) + [("empty2", 1, 0, 0)]
-        act += two("empty2", 0, 0) + two("empty2", 0, 1) + two("abs", 0) + [("empty2", 1, 0, 1)] + two("empty2", 1, 1)
-        pe += four("dh", 0) + [("turng", 1, 0)] + two("turnz", 0) + four("dh", 1) + products_first(w2(0, 2)) + means_first(w2(0, 3))
+        act += [("sort2", 0), ("sort2", 1)] + two("empty2", 0, 0) + two("empty2", 0, 1) + two("abs", 0) + [("empty2", 1, 0, 1)] + two("empty2", 1, 1)
+        pe += four("dh", 0) + [("turng", 1, 0)] + two("turnz", 0) + four("dh", 1) + products_first(w2(0, 2, "raw2")) + means_first(w2(0, 3, "raw2"))
         dve += four("mask", 0) + quant("w2", 1, 0) + quant("g", 1, 0) + [("mul2", 0, 2)] + dzn(0) + [("mul2", 0, 3), ("mul2", 1, 2)]
         act += two("emptyg", 1, 0) + two("emptyz", 0) + two("abs", 1) + two("empty2", 0, 2) + two("empty2", 0, 3)
 
-        pe += products_first(w2(1, 2)) + two("turnz", 1) + means_first(w2(1, 3)) + around(w1(0), w1(1))
-        dve += four("mask", 1) + [("mul1rest", 0), ("mul2", 1, 3)] + dzn(1) + [("mul1", 1)] + quant("w2", 0, 1) + dzh(0) + [("mul1", 2), ("mul1", 3)] + dzh(1)
+        pe += products_first(w2(1, 2, "raw2")) + two("turnz", 1) + means_first(w2(1, 3, "raw2")) + around(w1(0), w1(1))
+        dve += four("mask", 1) + [("mul1rest", 0), ("mul2", 1, 3), ("sort1", 0)] + dzn(1) + [("mul1", 1)] + quant("w2", 0, 1) + dzh(0) + [("mul1", 2), ("mul1", 3), ("sort1", 1)] + dzh(1)
         on_pool(("mul1most", 0), ("prod1", 0), ("gin", 1, 0))
         act += two("empty2", 1, 2) + two("abs", 2) + two("emptyz", 1) + two("empty2", 1, 3) + two("empty1", 0) + two("empty1", 1)
         pe += four("dh", 2) + around(w1(2), w1(3)) + two("turnz", 2) + open_with("mean1", 4) + [("turng", 0, 1)] + open_with("mean1", 5) + close_with("turn1", 4) + close_with("turn1", 5)
@@ -431,11 +487,11 @@ def tile_gaussian_nn_htanh_v_kernel(
         act += two("abs", 3) + two("empty1", 3) + two("emptyz", 2) + two("emptyg", 0, 1) + two("empty1", 4) + two("empty1", 5)
 
         pe += four("dh", 3) + around(w1(6), w1(7)) + two("turnz", 3) + open_with("mean1", 8) + [("turng", 1, 1)] + close_with("turn1", 8)
-        dve += four("mask", 3) + [("mul1rest", 8)] + dzn(3) + quant("g", 0, 1) + quant("w1", 0, 0) + two("weave", 0, 0) + quant("w1", 1, 0) + dzh(3)
+        dve += four("mask", 3) + [("mul1rest", 8), ("sort1", 2)] + dzn(3) + quant("g", 0, 1) + quant("w1", 0, 0) + two("weave", 0, 0) + quant("w1", 1, 0) + dzh(3)
         on_pool(("mul1most", 8), ("prod1", 8), ("dzin", 2))
         act += two("abs", 4) + two("empty1", 6) + two("empty1", 7) + two("emptyz", 3) + two("emptyg", 1, 1)
         pe += four("dh", 4) + four("dx", 0, 0)[:3] + two("turnz", 4) + means_first(w1(9)) + [("dx", 0, 0, 3)]
-        dve += four("mask", 4) + [("mul1rest", 9)] + quant("xq", 0, 0) + dzn(4) + quant("g", 1, 1) + two("weave", 1, 0) + quant("xq", 1, 0) + dzh(4)
+        dve += four("mask", 4) + [("mul1rest", 9)] + quant("xq", 0, 0) + dzn(4) + quant("g", 1, 1) + two("weave", 1, 0) + [("sort1", 3)] + quant("xq", 1, 0) + dzh(4)
         on_pool(("mul1most", 9), ("prod1", 9), ("dzin", 3))
         act += two("empty1", 8) + two("abs", 5) + four("emptyx", 0, 0)[:3] + two("emptyz", 4) + two("empty1", 9)
         pe += four("dh", 5) + dws("dw", 0, 0, range(4)) + two("turnz", 5) + around(w1(10), w1(11)) + dws("dw", 0, 1, range(4))
@@ -450,7 +506,7 @@ def tile_gaussian_nn_htanh_v_kernel(
         pool += [("flatmost", 14)]
         act += two("weave", 0, 1) + two("empty1", 12) + two("empty1", 13) + two("emptyz", 6) + two("abs", 7)
         pe += four("dh", 7) + dws("dw", 1, 0, range(4)) + two("turnz", 7) + dws("dw", 1, 0, range(4, 8)) + dws("dw", 1, 1, range(1))
-        dve += four("mask", 7) + dws("weigh", 1, 0, range(4)) + dzn(7) + dzh(6) + dzh(7) + [("add1", 14), ("add1", 15)]
+        dve += four("mask", 7) + dws("weigh", 1, 0, range(4)) + dzn(7) + dzh(6) + dzh(7) + [("add1s", 14), ("add1s", 15)]
         on_pool(("sum", 0, 0), ("total", 0, 0), ("dz", 6))
         pool += [("sum", 0, 1), ("sum", 0, 2), ("flatlow", 15)]
         act += two("emptyz", 7)
@@ -458,7 +514,7 @@ def tile_gaussian_nn_htanh_v_kernel(
         ring = [("dxbank", 1, 0, 0), ("dxbank", 1, 0, 1), ("w1words", 14), ("dxbank", 1, 0, 2), ("w1words", 15), ("dxbank", 1, 0, 3)]
         for n in range(3, len(ring)):
             inherits[ring[n]] = ring[n - 3]
-        pe += four("dx", 1, 0)[:2] + [("turn1w", 14), ("dx", 1, 0, 2), ("turn1w", 15), ("dx", 1, 0, 3)]
+        pe += four("dx", 1, 0)[:2] + [("turn1s", 14), ("dx", 1, 0, 2), ("turn1s", 15), ("dx", 1, 0, 3)]
         dve += dws("weigh", 1, 0, range(4, 8)) + dws("weigh", 1, 1, range(1)) + quant("w1", 0, 1) + quant("w1", 1, 1)
         act += four("emptyx", 1, 0)[:2] + [("empty1w", 14), ("emptyx", 1, 0, 2), ("empty1w", 15), ("emptyx", 1, 0, 3)]
         pe += dws("dw", 1, 1, range(1, 4))

@@ -21,6 +21,7 @@ BYTES = 2 * (N * X + 2 * X * H + J * X * H + 2 * H * Y + J * H * Y + J * N * Y) 
 P = 128
 T = 4
 K = P * T
+RUN = 8
 
 EDGE = 1.0 + 3.0 / 256.0
 
@@ -100,65 +101,56 @@ def tile_gaussian_nn_htanh_v_kernel(
                 specs[name] = ("bank", shape, F32)
             return names
 
-        def product(engine, out, noise, sig, places):
-            if engine is nc.gpsimd:
-                out, walk = out[:, places], lambda ap: ap.rearrange("p (m t) -> p t m", t=T)[:, places]
-            else:
-                out = out.rearrange("p t (w i) -> p w t i", i=2)[:, :, places]
-                walk = lambda ap: ap.rearrange("p (w i t) -> p w t i", t=T, i=2)[:, :, places]
-            engine.tensor_tensor(out=out, in0=walk(noise), in1=walk(sig), op=ALU.mult)
-
-        def sort_words(engine, out, mean):
-            copy(engine, out, mean.bitcast(F32).rearrange("p (m s) -> p s m", s=2))
-
-        def sorted_place(words, t):
-            return words[:, t // 2, :].bitcast(BF16).rearrange("p (m e) -> p e m", e=2)[:, t % 2, :]
-
-        shares = {"": (0, T), "most": (0, T - 1), "rest": (T - 1, T), "low": (0, 2), "high": (2, T)}
-
         def w2_load(src, name, a):
-            rows = src.rearrange("(q p u) y -> q p u y", q=2, u=T)
-            if a < 2:
-                load(name + (a,), "load", [P, 2, Y], BF16, rows[0][:, cols(a, 2), :])
-            else:
-                load(name + (2,), "load", [P, T, Y], BF16, rows[1])
+            blocks = 2 if a < 2 else 4
+            load(name + (min(a, 2),), "load", [P, blocks, Y], BF16, src.rearrange("(a b m) y -> a m b y", b=blocks, m=P)[a if a < 2 else 1])
 
         def w2_in(name, a):
-            return tiles[name + (min(a, 2),)][:, cols(max(a - 2, 0), 2), :].rearrange("p b y -> p (b y)")
+            return tiles[name + (min(a, 2),)][:, cols(max(a - 2, 0), 2), :]
 
         def w2_rows(a):
+            q, r = divmod(a, 2)
             for name, src in (("sig2", sig_W2), ("mu2", mu_W2)):
                 w2_load(src, (name,), a)
-            specs["mean2", a] = ("work", [P, 2, 2 * P], F32)
-            step(("sort2", a), [("mu2", min(a, 2))], [("mean2", a)], lambda engine: sort_words(engine, tiles["mean2", a][:], w2_in(("mu2",), a)))
+            specs["mean2", a] = ("work", [P, T, 2, P], BF16)
+
+            def sort_mean(engine):
+                src = w2_in(("mu2",), a).rearrange("p b (w i t) -> p (b w) t i", t=T, i=4)
+                copy(engine, tiles["mean2", a][:].rearrange("p t b (w i) -> p (b w) t i", i=4), src)
+
+            step(("sort2", a), [("mu2", min(a, 2))], [("mean2", a)], sort_mean)
             for j in range(J):
-                w2_sample(j, a, *divmod(a, 2))
+                w2_sample(j, a, q, r)
 
         def w2_sample(j, a, q, r):
             w2_load(e_W2[j], ("e2", j), a)
-            specs["prod2", j, a] = ("work", [P, T, 2 * P], F32)
+            specs["prod2", j, a] = ("work", [P, T, 2, P], F32)
             specs["w2in", j, q] = ("work", [P, K, T], BF16)
             banks = banks_for(("w2bank", j, a), 2, [P, T, P])
 
             def multiply(places, engine):
-                product(engine, tiles["prod2", j, a][:], w2_in(("e2", j), a), w2_in(("sig2",), a), places)
+                if engine is nc.gpsimd:
+                    out = tiles["prod2", j, a][:].rearrange("p t b w -> p t (b w)")[:, places]
+                    noise, sig = (w2_in(name, a).rearrange("p b (w t) -> p t (b w)", t=T)[:, places] for name in (("e2", j), ("sig2",)))
+                else:
+                    out = tiles["prod2", j, a][:].rearrange("p t b (w i) -> p (b w) t i", i=2)[:, :, places]
+                    noise, sig = (w2_in(name, a).rearrange("p b (w i t) -> p (b w) t i", t=T, i=2)[:, :, places] for name in (("e2", j), ("sig2",)))
+                engine.tensor_tensor(out=out, in0=noise, in1=sig, op=ALU.mult)
 
-            def turn(is_mean, first, engine):
-                block = w2_in(("mu2",), a).rearrange("p (m t) -> p t m", t=T) if is_mean else tiles["prod2", j, a][:]
-                turn_part(banks, lambda b, t: block[:, t, cols(b)], is_mean, first)
-
-            def turn_sorted(first, engine):
-                turn_part(banks, lambda b, t: sorted_place(tiles["mean2", a][:], t)[:, cols(b)], True, first)
+            def turn(source, first, engine):
+                block = w2_in(("mu2",), a).rearrange("p b (w t) -> p t b w", t=T) if source[0] == "mu2" else tiles[source]
+                turn_part(banks, lambda b, t: block[:, t, b, :], source[0] != "prod2", first)
 
             def empty(b, engine):
-                copy(engine, tiles["w2in", j, q][:, cols(2 * r + b), :], tiles[banks[b]][:].rearrange("p t m -> p m t"))
+                dst = tiles["w2in", j, q][:].rearrange("p (u b i) t -> p u b i t", u=T, i=RUN)
+                src = tiles[banks[b]][:].rearrange("p t (b u i) -> p u b i t", u=T, i=RUN)
+                copy(engine, dst[:, :, cols(2 * r + b, 4), :, :], src)
 
-            for name, places in shares.items():
-                step(("mul2" + name, j, a), [("e2", j, min(a, 2)), ("sig2", min(a, 2))], [("prod2", j, a)], partial(multiply, slice(*places)))
+            for name, places in {"mul2": (0, T), "mul2most": (0, T - 1), "mul2rest": (T - 1, T), "mul2low": (0, 2), "mul2high": (2, T)}.items():
+                step((name, j, a), [("e2", j, min(a, 2)), ("sig2", min(a, 2))], [("prod2", j, a)], partial(multiply, slice(*places)))
             for first in (False, True):
-                step(("turn2", j, a, first), [("prod2", j, a)], banks, partial(turn, False, first))
-                step(("raw2", j, a, first), [("mu2", min(a, 2))], banks, partial(turn, True, first))
-                step(("mean2", j, a, first), [("mean2", a)], banks, partial(turn_sorted, first))
+                for name, source in (("turn2", ("prod2", j, a)), ("mean2", ("mean2", a)), ("raw2", ("mu2", min(a, 2)))):
+                    step((name, j, a, first), [source], banks, partial(turn, source, first))
             for b in range(2):
                 step(("empty2", j, a, b), [banks[b]], [("w2in", j, q)], partial(empty, b))
             quantize(("w2", j, q), E4M3, ("w2in", j, q))
@@ -200,8 +192,12 @@ def tile_gaussian_nn_htanh_v_kernel(
         def w1_pair(a):
             for name, src in ((("sig1",), sig_W1), (("mu1",), mu_W1), (("e1", 0), e_W1[0]), (("e1", 1), e_W1[1])):
                 load(name + (a,), "load", [P, 2, H], BF16, src.rearrange("(a m r) h -> a m r h", r=2, m=P)[a])
-            specs["mean1", a] = ("work", [P, 2, K], F32)
-            step(("sort1", a), [("mu1", a)], [("mean1", a)], lambda engine: sort_words(engine, tiles["mean1", a][:], tiles["mu1", a][:].rearrange("p r h -> p (r h)")))
+            specs["mean1", a] = ("work", [P, 2, T, 32, RUN], BF16)
+
+            def sort_mean(engine):
+                copy(engine, tiles["mean1", a][:], tiles["mu1", a][:].rearrange("p r (b u i) -> p r u b i", u=T, i=RUN))
+
+            step(("sort1", a), [("mu1", a)], [("mean1", a)], sort_mean)
             for i in (2 * a, 2 * a + 1):
                 for j in range(J):
                     w1_block(i, j)
@@ -210,52 +206,56 @@ def tile_gaussian_nn_htanh_v_kernel(
             a, r = divmod(i, 2)
             xh, c = divmod(i, 4)
             n = 4 * a + 2 * j + r
-            specs["prod1", n] = ("work", [P, T, 2 * P], F32)
-            specs["flat1", n] = ("work", [P, H], F32)
-            specs["sum1", n] = ("work", [P, H], BF16)
+            specs["prod1", n] = ("work", [P, T, 32, RUN], F32)
+            specs["sum1", n] = ("work", [P, 2, 2 * P, 2], BF16)
             specs["w1in", j, xh] = ("w1in", [P, 2 * K, T], BF16)
             banks = banks_for(("w1bank", n), 2, [P, T, P])
             specs["w1words", n] = ("bank", [P, 2, 2, P], F32)
 
             def multiply(places, engine):
-                product(engine, tiles["prod1", n][:], tiles["e1", j, a][:, r, :], tiles["sig1", a][:, r, :], places)
+                sort = "p (b u i) -> p u b i"
+                engine.tensor_tensor(
+                    out=tiles["prod1", n][:, places],
+                    in0=tiles["e1", j, a][:, r, :].rearrange(sort, u=T, i=RUN)[:, places],
+                    in1=tiles["sig1", a][:, r, :].rearrange(sort, u=T, i=RUN)[:, places],
+                    op=ALU.mult,
+                )
 
             def turn(is_mean, first, engine):
-                block = tiles["mu1", a][:, r, :].rearrange("p (m u) -> p u m", u=T) if is_mean else tiles["prod1", n][:]
-                turn_part(banks, lambda q, u: block[:, u, cols(q)], is_mean, first)
-
-            def turn_sorted(first, engine):
-                turn_part(banks, lambda q, u: sorted_place(tiles["mean1", a][:], u)[:, cols(2 * r + q)], True, first)
+                block = (tiles["mean1", a][:, r] if is_mean else tiles["prod1", n][:]).rearrange("p u (q b) i -> p u q (b i)", q=2)
+                turn_part(banks, lambda q, u: block[:, u, q, :], is_mean, first)
 
             def empty(q, engine):
                 copy(engine, tiles["w1in", j, xh][:, cols(T * q + c), :], tiles[banks[q]][:].rearrange("p u m -> p m u"))
 
-            def multiply_flat(part, engine):
-                engine.tensor_tensor(out=tiles["flat1", n][:, part], in0=tiles["e1", j, a][:, r, part], in1=tiles["sig1", a][:, r, part], op=ALU.mult)
-
             def add_mean(engine):
-                engine.tensor_tensor(out=tiles["sum1", n][:], in0=tiles["flat1", n][:], in1=tiles["mu1", a][:, r, :], op=ALU.add)
-
-            def add_sorted(engine):
-                walk = "p (m s e) -> p m s e"
+                pair = "p (s e) b i -> p s (b i) e"
                 engine.tensor_tensor(
-                    out=tiles["sum1", n][:].rearrange("p (s m e) -> p m s e", s=2, e=2),
-                    in0=tiles["flat1", n][:].rearrange(walk, s=2, e=2),
-                    in1=tiles["mu1", a][:, r, :].rearrange(walk, s=2, e=2),
+                    out=tiles["sum1", n][:],
+                    in0=tiles["prod1", n][:].rearrange(pair, e=2),
+                    in1=tiles["mean1", a][:, r].rearrange(pair, e=2),
                     op=ALU.add,
                 )
 
-            def turn_sorted_words(engine):
-                words = tiles["sum1", n][:].bitcast(F32).rearrange("p (s q m) -> p q s m", s=2, q=2)
-                for q in range(2):
-                    for s in range(2):
-                        engine.transpose(tiles["w1words", n][:, q, s, :], words[:, q, s, :], ident_f[:])
+            def multiply_flat(part, engine):
+                engine.tensor_tensor(out=tiles["flat1", n][:, part], in0=tiles["e1", j, a][:, r, part], in1=tiles["sig1", a][:, r, part], op=ALU.mult)
 
-            step(("add1s", n), [("flat1", n), ("mu1", a)], [("sum1", n)], add_sorted)
-            step(("turn1s", n), [("sum1", n)], [("w1words", n)], turn_sorted_words)
+            def add_raw(engine):
+                pair = "p (b s e i) -> p b s i e"
+                engine.tensor_tensor(
+                    out=tiles["sum1", n][:].rearrange("p s (b i) e -> p b s i e", i=RUN),
+                    in0=tiles["flat1", n][:].rearrange(pair, s=2, e=2, i=RUN),
+                    in1=tiles["mu1", a][:, r, :].rearrange(pair, s=2, e=2, i=RUN),
+                    op=ALU.add,
+                )
+
+            specs["flat1", n] = ("work", [P, H], F32)
+            for name, part in {"flat": (0, 4), "flatmost": (0, 3), "flatrest": (3, 4), "flatlow": (0, 2), "flathigh": (2, 4)}.items():
+                step((name, n), [("e1", j, a), ("sig1", a)], [("flat1", n)], partial(multiply_flat, slice(2 * P * part[0], 2 * P * part[1])))
+            step(("addraw", n), [("flat1", n), ("mu1", a)], [("sum1", n)], add_raw)
 
             def turn_words(engine):
-                words = tiles["sum1", n][:].bitcast(F32).rearrange("p (q m s) -> p q s m", s=2, q=2)
+                words = tiles["sum1", n][:].rearrange("p s m e -> p (s m e)").bitcast(F32).rearrange("p (s q m) -> p q s m", s=2, q=2)
                 for q in range(2):
                     for s in range(2):
                         engine.transpose(tiles["w1words", n][:, q, s, :], words[:, q, s, :], ident_f[:])
@@ -264,16 +264,15 @@ def tile_gaussian_nn_htanh_v_kernel(
                 dst = tiles["w1in", j, xh][:].rearrange("p c t -> p (c t)").bitcast(F32).rearrange("p (q c m s) -> p q c m s", q=2, m=P, s=2)
                 copy(engine, dst[:, :, c], tiles["w1words", n][:].rearrange("p q s m -> p q m s"))
 
+            shares = {"mul1": (0, T), "mul1most": (0, T - 1), "mul1rest": (T - 1, T), "mul1low": (0, 2), "mul1high": (2, T)}
             for name, places in shares.items():
-                step(("mul1" + name, n), [("e1", j, a), ("sig1", a)], [("prod1", n)], partial(multiply, slice(*places)))
-                step(("flat" + name, n), [("e1", j, a), ("sig1", a)], [("flat1", n)], partial(multiply_flat, slice(2 * P * places[0], 2 * P * places[1])))
+                step((name, n), [("e1", j, a), ("sig1", a)], [("prod1", n)], partial(multiply, slice(*places)))
             for first in (False, True):
                 step(("turn1", n, first), [("prod1", n)], banks, partial(turn, False, first))
-                step(("raw1", n, first), [("mu1", a)], banks, partial(turn, True, first))
-                step(("mean1", n, first), [("mean1", a)], banks, partial(turn_sorted, first))
+                step(("mean1", n, first), [("mean1", a)], banks, partial(turn, True, first))
             for q in range(2):
                 step(("empty1", n, q), [banks[q]], [("w1in", j, xh)], partial(empty, q))
-            step(("add1", n), [("flat1", n), ("mu1", a)], [("sum1", n)], add_mean)
+            step(("add1", n), [("prod1", n), ("mean1", a)], [("sum1", n)], add_mean)
             step(("turn1w", n), [("sum1", n)], [("w1words", n)], turn_words)
             step(("empty1w", n), [("w1words", n)], [("w1in", j, xh)], empty_words)
             quantize(("w1", j, xh), E4M3, ("w1in", j, xh), kind="wide")
@@ -287,8 +286,8 @@ def tile_gaussian_nn_htanh_v_kernel(
             turned = banks_for(("dzbank", k), 2, [P, T, P])
 
             def absolute(part, engine):
-                dst = tiles["abs", k][:, part, :].rearrange("p (c i) t -> p c t i", i=4)
-                src = tiles["z", k][:, :, part].rearrange("p t (c i) -> p c t i", i=4)
+                dst = tiles["abs", k][:, part, :].rearrange("p (c i) t -> p c t i", i=2)
+                src = tiles["z", k][:, :, part].rearrange("p t (c i) -> p c t i", i=2)
                 engine.activation(out=dst, in_=src, func=ACT.Abs, scale=EDGE)
 
             def multiply(u, engine):
@@ -296,43 +295,39 @@ def tile_gaussian_nn_htanh_v_kernel(
                     mx(tiles[dh[u]][:, t, :], ("g", j, g), cols(t), E5M2, ("w2", j, q), cols(u), E4M3, True, True)
 
             def mask(u, engine):
-                size = tiles["abs", k][:].rearrange("p (m u) t -> p u m t", u=T)
-                bank = tiles[dh[u]][:].rearrange("p t m -> p m t")
-                engine.scalar_tensor_tensor(out=tiles["dz", k][:, cols(u), :], in0=size[:, u], scalar=EDGE, in1=bank, op0=ALU.is_lt, op1=ALU.mult)
+                dz = tiles["dz", k][:].rearrange("p (u b i) t -> p u b i t", u=T, i=RUN)
+                size = tiles["abs", k][:].rearrange("p (b u i) t -> p u b i t", u=T, i=RUN)
+                bank = tiles[dh[u]][:].rearrange("p t (b i) -> p b i t", i=RUN)
+                engine.scalar_tensor_tensor(out=dz[:, u], in0=size[:, u], scalar=EDGE, in1=bank, op0=ALU.is_lt, op1=ALU.mult)
 
             def turn(s, engine):
                 words = tiles["dz", k][:].rearrange("p c t -> p (c t)").bitcast(F32).rearrange("p (u m s) -> p s u m", u=T, s=2)
                 for u in range(T):
                     engine.transpose(tiles[turned[s]][:, u, :], words[:, s, u, :], ident_f[:])
 
+            specs["dzs", k] = ("work", [P, 2, T, P], F32)
+
+            def sort_words(engine):
+                words = tiles["dz", k][:].rearrange("p c t -> p (c t)").bitcast(F32).rearrange("p (c m s) -> p c s m", m=4, s=2)
+                copy(engine, tiles["dzs", k][:].rearrange("p s u (c m) -> p (u c) s m", m=4), words)
+
+            def turn_sorted(s, engine):
+                for u in range(T):
+                    engine.transpose(tiles[turned[s]][:, u, :], tiles["dzs", k][:, s, u, :], ident_f[:])
+
+            step(("sortz", k), [("dz", k)], [("dzs", k)], sort_words)
+            for n in range(2):
+                step(("turnzs", k, n), [("dzs", k)], [turned[n]], partial(turn_sorted, n))
+
             def empty(s, engine):
                 src = tiles[turned[s]][:].bitcast(BF16).rearrange("p u (m e) -> p e m u", e=2)
                 copy(engine, tiles["dzin", k][:, cols(s, K // 2), :].rearrange("p (e m) u -> p e m u", e=2), src)
 
-            specs["dzs", k] = ("work", [P, 2, K], F32)
-
-            def turn_sorted(s, engine):
-                for u in range(T):
-                    engine.transpose(tiles[turned[s]][:, u, :], tiles["dzs", k][:, s, cols(u)], ident_f[:])
-
-            step(("sortz", k), [("dz", k)], [("dzs", k)], lambda engine: sort_words(engine, tiles["dzs", k][:], tiles["dz", k][:].rearrange("p c t -> p (c t)")))
-            for n in range(2):
-                step(("turnzs", k, n), [("dzs", k)], [turned[n]], partial(turn_sorted, n))
-            zview = z1[j].rearrange("(g p t) h -> g p t h", g=2, t=T)[g]
-
-            def absolute_half(n, engine):
-                dst = tiles["abs", k][:, cols(n, K // 2), :].rearrange("p (c i) t -> p c t i", i=4)
-                src = tiles["zhalf", k, n][:].rearrange("p t (c i) -> p c t i", i=4)
-                engine.activation(out=dst, in_=src, func=ACT.Abs, scale=EDGE)
-
-            for n in range(2):
-                load(("zhalf", k, n), "load", [P, T, K // 2], F32, zview[:, :, cols(2 * q + n, K // 2)])
-                step(("abshalf", k, n), [("zhalf", k, n)], [("abs", k)], partial(absolute_half, n))
-            step(("abs", k), [("z", k)], [("abs", k)], partial(absolute, cols(0, K)))
             for n in range(2):
                 step(("abs", k, n), [("z", k)], [("abs", k)], partial(absolute, cols(n, K // 2)))
                 step(("turnz", k, n), [("dz", k)], [turned[n]], partial(turn, n))
                 step(("emptyz", k, n), [turned[n]], [("dzin", k)], partial(empty, n))
+            step(("abs", k), [("z", k)], [("abs", k)], partial(absolute, cols(0, K)))
             for u in range(T):
                 step(("dh", k, u), [("g", j, g), ("w2", j, q)], [dh[u]], partial(multiply, u))
                 step(("mask", k, u), [("abs", k), dh[u]], [("dz", k)], partial(mask, u))
@@ -369,6 +364,7 @@ def tile_gaussian_nn_htanh_v_kernel(
             part = ("part", q, i // 2, j)
             specs[bank] = ("bank", [P, K], F32)
             specs[part] = ("work", [P, 2, K], F32)
+            natural = "p (b u i) -> p b u i"
 
             def multiply(engine):
                 for g in range(2):
@@ -376,9 +372,9 @@ def tile_gaussian_nn_htanh_v_kernel(
 
             def weigh(engine):
                 engine.tensor_tensor(
-                    out=tiles[part][:, i % 2, :].rearrange("p (m u) -> p m u", u=T),
-                    in0=tiles["e1", j, i // 2][:, i % 2, cols(q, K)].rearrange("p (m u) -> p m u", u=T),
-                    in1=tiles[bank][:].rearrange("p (u m) -> p m u", u=T),
+                    out=tiles[part][:, i % 2, :].rearrange(natural, u=T, i=RUN),
+                    in0=tiles["e1", j, i // 2][:, i % 2, cols(q, K)].rearrange(natural, u=T, i=RUN),
+                    in1=tiles[bank][:].rearrange("p (u b i) -> p b u i", u=T, i=RUN),
                     op=ALU.mult,
                 )
 
@@ -452,8 +448,8 @@ def tile_gaussian_nn_htanh_v_kernel(
         def w2(j, a, mean):
             return (("turn2", j, a), (mean, j, a))
 
-        def w1(n, mean="mean1"):
-            return (("turn1", n), (mean, n))
+        def w1(n):
+            return (("turn1", n), ("mean1", n))
 
         def products_first(*jobs):
             return [job[0] + (True,) for job in jobs] + [job[1] + (False,) for job in jobs]
@@ -475,46 +471,46 @@ def tile_gaussian_nn_htanh_v_kernel(
         act += [("sort2", 0), ("sort2", 1)] + two("empty2", 0, 0) + two("empty2", 0, 1) + two("abs", 0) + [("empty2", 1, 0, 1)] + two("empty2", 1, 1)
         pe += four("dh", 0) + [("turng", 1, 0)] + two("turnz", 0) + four("dh", 1) + products_first(w2(0, 2, "raw2")) + means_first(w2(0, 3, "raw2"))
         dve += four("mask", 0) + quant("w2", 1, 0) + quant("g", 1, 0) + [("mul2", 0, 2)] + dzn(0) + [("mul2", 0, 3), ("mul2", 1, 2)]
-        act += two("emptyg", 1, 0) + two("emptyz", 0) + two("abs", 1) + two("empty2", 0, 2) + two("empty2", 0, 3)
+        act += two("emptyg", 1, 0) + two("emptyz", 0) + [("abs", 1)] + two("empty2", 0, 2) + two("empty2", 0, 3)
 
         pe += products_first(w2(1, 2, "raw2")) + two("turnz", 1) + means_first(w2(1, 3, "raw2")) + around(w1(0), w1(1))
         dve += four("mask", 1) + [("mul1rest", 0), ("mul2", 1, 3), ("sort1", 0)] + dzn(1) + [("mul1", 1)] + quant("w2", 0, 1) + dzh(0) + [("mul1", 2), ("mul1", 3), ("sort1", 1)] + dzh(1)
         on_pool(("mul1most", 0), ("prod1", 0), ("gin", 1, 0))
-        act += two("empty2", 1, 2) + two("abs", 2) + two("emptyz", 1) + two("empty2", 1, 3) + two("empty1", 0) + two("empty1", 1)
+        act += two("empty2", 1, 2) + [("abs", 2)] + two("emptyz", 1) + two("empty2", 1, 3) + two("empty1", 0) + two("empty1", 1)
         pe += four("dh", 2) + around(w1(2), w1(3)) + two("turnz", 2) + open_with("mean1", 4) + [("turng", 0, 1)] + open_with("mean1", 5) + close_with("turn1", 4) + close_with("turn1", 5)
         dve += four("mask", 2) + two("empty1", 2) + [("mul1", 5)] + quant("w2", 1, 1) + dzn(2) + [("mul1", 6), ("mul1", 7)] + dzh(2)
         on_pool(("mul1", 4), ("prod1", 4), ("dzin", 1))
-        act += two("abs", 3) + two("empty1", 3) + two("emptyz", 2) + two("emptyg", 0, 1) + two("empty1", 4) + two("empty1", 5)
+        act += [("abs", 3)] + two("empty1", 3) + two("emptyz", 2) + two("emptyg", 0, 1) + two("empty1", 4) + two("empty1", 5)
 
         pe += four("dh", 3) + around(w1(6), w1(7)) + two("turnz", 3) + open_with("mean1", 8) + [("turng", 1, 1)] + close_with("turn1", 8)
         dve += four("mask", 3) + [("mul1rest", 8), ("sort1", 2)] + dzn(3) + quant("g", 0, 1) + quant("w1", 0, 0) + two("weave", 0, 0) + quant("w1", 1, 0) + dzh(3)
         on_pool(("mul1most", 8), ("prod1", 8), ("dzin", 2))
-        act += two("abs", 4) + two("empty1", 6) + two("empty1", 7) + two("emptyz", 3) + two("emptyg", 1, 1)
+        act += [("abs", 4)] + two("empty1", 6) + two("empty1", 7) + two("emptyz", 3) + two("emptyg", 1, 1)
         pe += four("dh", 4) + four("dx", 0, 0)[:3] + two("turnz", 4) + means_first(w1(9)) + [("dx", 0, 0, 3)]
         dve += four("mask", 4) + [("mul1rest", 9)] + quant("xq", 0, 0) + dzn(4) + quant("g", 1, 1) + two("weave", 1, 0) + [("sort1", 3)] + quant("xq", 1, 0) + dzh(4)
         on_pool(("mul1most", 9), ("prod1", 9), ("dzin", 3))
-        act += two("empty1", 8) + two("abs", 5) + four("emptyx", 0, 0)[:3] + two("emptyz", 4) + two("empty1", 9)
+        act += two("empty1", 8) + [("abs", 5)] + four("emptyx", 0, 0)[:3] + two("emptyz", 4) + two("empty1", 9)
         pe += four("dh", 5) + dws("dw", 0, 0, range(4)) + two("turnz", 5) + around(w1(10), w1(11)) + dws("dw", 0, 1, range(4))
         dve += four("mask", 5) + dws("weigh", 0, 0, range(4)) + [("mul1rest", 11)] + dzn(5) + [("mul1", 12)] + dzh(5) + dws("weigh", 0, 1, range(4))
         on_pool(("mul1", 10), ("prod1", 10), ("dzin", 4))
         pool.append(("mul1most", 11))
-        act += [("emptyx", 0, 0, 3)] + two("weave", 1, 1) + two("emptyz", 5) + two("abs", 6) + two("empty1", 10) + two("empty1", 11)
+        act += [("emptyx", 0, 0, 3)] + two("weave", 1, 1) + two("emptyz", 5) + [("abs", 6)] + two("empty1", 10) + two("empty1", 11)
 
         pe += four("dh", 6) + around(w1(12), w1(13)) + two("turnz", 6) + dws("dw", 0, 0, range(4, 8)) + dws("dw", 0, 1, range(4, 8))
-        dve += four("mask", 6) + [("flatrest", 14)] + quant("xq", 1, 1) + quant("xq", 0, 1) + [("flathigh", 15)] + dzn(6) + dws("weigh", 0, 0, range(4, 8)) + dws("weigh", 0, 1, range(4, 8))
+        dve += four("mask", 6) + [("mul1rest", 14)] + quant("xq", 1, 1) + quant("xq", 0, 1) + [("mul1high", 15)] + dzn(6) + dws("weigh", 0, 0, range(4, 8)) + dws("weigh", 0, 1, range(4, 8))
         on_pool(("mul1", 13), ("prod1", 13), ("dzin", 5))
-        pool += [("flatmost", 14)]
-        act += two("weave", 0, 1) + two("empty1", 12) + two("empty1", 13) + two("emptyz", 6) + two("abs", 7)
+        pool += [("mul1most", 14)]
+        act += two("weave", 0, 1) + two("empty1", 12) + two("empty1", 13) + two("emptyz", 6) + [("abs", 7)]
         pe += four("dh", 7) + dws("dw", 1, 0, range(4)) + two("turnz", 7) + dws("dw", 1, 0, range(4, 8)) + dws("dw", 1, 1, range(1))
-        dve += four("mask", 7) + dws("weigh", 1, 0, range(4)) + dzn(7) + dzh(6) + dzh(7) + [("add1s", 14), ("add1s", 15)]
+        dve += four("mask", 7) + dws("weigh", 1, 0, range(4)) + dzn(7) + dzh(6) + dzh(7) + [("add1", 14), ("add1", 15)]
         on_pool(("sum", 0, 0), ("total", 0, 0), ("dz", 6))
-        pool += [("sum", 0, 1), ("sum", 0, 2), ("flatlow", 15)]
+        pool += [("sum", 0, 1), ("sum", 0, 2), ("mul1low", 15)]
         act += two("emptyz", 7)
         sp += four("store1", 0)[:3]
         ring = [("dxbank", 1, 0, 0), ("dxbank", 1, 0, 1), ("w1words", 14), ("dxbank", 1, 0, 2), ("w1words", 15), ("dxbank", 1, 0, 3)]
         for n in range(3, len(ring)):
             inherits[ring[n]] = ring[n - 3]
-        pe += four("dx", 1, 0)[:2] + [("turn1s", 14), ("dx", 1, 0, 2), ("turn1s", 15), ("dx", 1, 0, 3)]
+        pe += four("dx", 1, 0)[:2] + [("turn1w", 14), ("dx", 1, 0, 2), ("turn1w", 15), ("dx", 1, 0, 3)]
         dve += dws("weigh", 1, 0, range(4, 8)) + dws("weigh", 1, 1, range(1)) + quant("w1", 0, 1) + quant("w1", 1, 1)
         act += four("emptyx", 1, 0)[:2] + [("empty1w", 14), ("emptyx", 1, 0, 2), ("empty1w", 15), ("emptyx", 1, 0, 3)]
         pe += dws("dw", 1, 1, range(1, 4))
@@ -523,7 +519,7 @@ def tile_gaussian_nn_htanh_v_kernel(
         pe += four("dx", 1, 1)[:3] + two("dx", 1, 1, T - 1)
         dve += dws("weigh", 1, 1, range(1, 6)) + [("sum", 1, 1), ("sum", 1, 2)] + dws("weigh", 1, 1, range(6, 8)) + [("sum", 1, 3)]
         pool += [("sum", 0, 3), ("sum", 1, 0)]
-        inherits["total", 0, 3] = ("flat1", 15)
+        inherits["total", 0, 3] = ("prod1", 15)
         act += four("emptyx", 0, 1) + four("emptyx", 1, 1)[:3] + [("emptyx", 1, 1, 3, 0)]
         dve.append(("emptyx", 1, 1, 3, 1))
         sp += four("store0", 1, 0)[:2] + [("store1", 0, 3)] + four("store0", 1, 0)[2:]

@@ -27,6 +27,7 @@ EDGE = 1.0 + 3.0 / 256.0
 
 UNITS = [(j, q, g) for g in range(2) for q in range(2) for j in range(J)]
 
+SHIFT = 128
 SLOTS = {"load": 13, "work": 17, "z": 3, "w1in": 2, "code": 22, "wide": 4, "bank": 8}
 
 
@@ -39,9 +40,9 @@ def tile_gaussian_nn_htanh_v_kernel(
         sbuf = ctx.enter_context(tc.tile_pool(name="sbuf", bufs=1))
         psum = ctx.enter_context(tc.psum_pool(name="psum", bufs=1))
 
-        ident_f = sbuf.tile([P, P], F32, name="ident_f", tag="ident_f")
+        ident_f = sbuf.tile([P, P], F32, name="ident_f", tag="ident_f", align_bytes=256, offset=0)
         make_identity(nc, ident_f[:])
-        ident_b = sbuf.tile([P, P], BF16, name="ident_b", tag="ident_b")
+        ident_b = sbuf.tile([P, P], BF16, name="ident_b", tag="ident_b", align_bytes=256, offset=512)
         nc.vector.tensor_copy(out=ident_b[:], in_=ident_f[:])
         ctx.enter_context(tc.manual_schedule())
 
@@ -551,6 +552,16 @@ def tile_gaussian_nn_htanh_v_kernel(
                 and all(key in slots for key in fresh(name) if key in inherits)
             )
 
+        sizes = {"load": 4096, "work": 4096, "z": 8192, "w1in": 8192, "code": 2048 + SHIFT, "code_s": 512, "wide": 4096, "wide_s": 1024}
+        begins = {}
+        place = 768
+        for kind, size in sizes.items():
+            begins[kind] = place
+            place = place + size * SLOTS[kind.replace("_s", "")]
+
+        def offset(kind, slot):
+            return begins[kind] + sizes[kind] * slot
+
         def take(key):
             kind, shape, dtype = specs[key]
             if key not in inherits:
@@ -559,11 +570,14 @@ def tile_gaussian_nn_htanh_v_kernel(
             if kind == "bank":
                 tiles[key] = psum.tile(shape, dtype, name=key[0], tag=tag)
             elif kind in ("code", "wide"):
-                words = sbuf.tile(shape, U32, name=key[0], tag=tag, align_bytes=64)
-                scales = sbuf.tile(shape, U8, name=key[0] + "_s", tag=tag + "_s", align_bytes=64)
+                at = offset(*slots[key])
+                if kind == "code":
+                    at = at + (SHIFT if (at % 256 == 0) == (key[0] in ("g", "dzh", "xq")) else 0)
+                words = sbuf.tile(shape, U32, name=key[0], tag="%s_%d" % (kind, at), align_bytes=64, offset=at)
+                scales = sbuf.tile(shape, U8, name=key[0] + "_s", tag=tag + "_s", align_bytes=64, offset=offset(kind + "_s", slots[key][1]))
                 tiles[key] = (words, scales)
             else:
-                tiles[key] = sbuf.tile(shape, dtype, name=key[0], tag=tag, align_bytes=64)
+                tiles[key] = sbuf.tile(shape, dtype, name=key[0], tag=tag, align_bytes=64, offset=offset(*slots[key]))
 
         def emit(engine, name):
             reads, writes, work = steps[name]

@@ -40,9 +40,9 @@ def tile_gaussian_nn_htanh_v_kernel(
         sbuf = ctx.enter_context(tc.tile_pool(name="sbuf", bufs=1))
         psum = ctx.enter_context(tc.psum_pool(name="psum", bufs=1))
 
-        ident_f = sbuf.tile([P, P], F32, name="ident_f", tag="ident_f", align_bytes=256, offset=0)
+        ident_f = sbuf.tile([P, P], F32, name="ident_f", tag="ident_f", align_bytes=64, offset=128)
         make_identity(nc, ident_f[:])
-        ident_b = sbuf.tile([P, P], BF16, name="ident_b", tag="ident_b", align_bytes=256, offset=512)
+        ident_b = sbuf.tile([P, P], BF16, name="ident_b", tag="ident_b", align_bytes=64, offset=640)
         nc.vector.tensor_copy(out=ident_b[:], in_=ident_f[:])
         ctx.enter_context(tc.manual_schedule())
 
@@ -552,11 +552,11 @@ def tile_gaussian_nn_htanh_v_kernel(
                 and all(key in slots for key in fresh(name) if key in inherits)
             )
 
-        sizes = {"load": 4096, "work": 4096, "z": 8192, "w1in": 8192, "code": 2048 + SHIFT, "code_s": 512, "wide": 4096, "wide_s": 1024}
+        sizes = {"load": 4096, "work": 4096, "z": 8192, "w1in": 8192, "code": 2048 + SHIFT, "wide": 4096, "code_s": 512, "wide_s": 1024}
         begins = {}
-        place = 768
+        place = 1024
         for kind, size in sizes.items():
-            begins[kind] = place
+            begins[kind] = place + (64 if kind in ("code_s", "wide_s") else 0)
             place = place + size * SLOTS[kind.replace("_s", "")]
 
         def offset(kind, slot):
@@ -577,7 +577,7 @@ def tile_gaussian_nn_htanh_v_kernel(
                 scales = sbuf.tile(shape, U8, name=key[0] + "_s", tag=tag + "_s", align_bytes=64, offset=offset(kind + "_s", slots[key][1]))
                 tiles[key] = (words, scales)
             else:
-                tiles[key] = sbuf.tile(shape, dtype, name=key[0], tag=tag, align_bytes=64, offset=offset(*slots[key]))
+                tiles[key] = sbuf.tile(shape, dtype, name=key[0], tag=tag, align_bytes=256, offset=offset(*slots[key]))
 
         def emit(engine, name):
             reads, writes, work = steps[name]

@@ -199,6 +199,19 @@ def tile_gaussian_nn_htanh_v_kernel(
                 copy(engine, tiles["mean1", a][:], tiles["mu1", a][:].rearrange("p r (b u i) -> p r u b i", u=T, i=RUN))
 
             step(("sort1", a), [("mu1", a)], [("mean1", a)], sort_mean)
+
+            def sort_row(engine):
+                copy(engine, tiles["mean1", a][:, 0], tiles["mu1", a][:, 0, :].rearrange("p (b u i) -> p u b i", u=T, i=RUN))
+
+            step(("sort1row", a), [("mu1", a)], [("mean1", a)], sort_row)
+
+            def lay_sig(r, engine):
+                for half in range(2):
+                    engine.matmul(tiles["sigbank", a, r][:, cols(half, K)], lhsT=ident_b[:], rhs=tiles["sig1", a][:, r, cols(half, K)], start=True, stop=True)
+
+            for r in range(2):
+                specs["sigbank", a, r] = ("bank", [P, H], BF16)
+                step(("laysig", a, r), [("sig1", a)], [("sigbank", a, r)], partial(lay_sig, r))
             for i in (2 * a, 2 * a + 1):
                 for j in range(J):
                     w1_block(i, j)
@@ -221,6 +234,17 @@ def tile_gaussian_nn_htanh_v_kernel(
                     in1=tiles["sig1", a][:, r, :].rearrange(sort, u=T, i=RUN)[:, places],
                     op=ALU.mult,
                 )
+
+            def multiply_bank(engine):
+                sort = "p (b u i) -> p u b i"
+                engine.tensor_tensor(
+                    out=tiles["prod1", n][:],
+                    in0=tiles["e1", j, a][:, r, :].rearrange(sort, u=T, i=RUN),
+                    in1=tiles["sigbank", a, r][:].rearrange(sort, u=T, i=RUN),
+                    op=ALU.mult,
+                )
+
+            step(("mul1p", n), [("e1", j, a), ("sigbank", a, r)], [("prod1", n)], multiply_bank)
 
             def turn(is_mean, first, engine):
                 block = (tiles["mean1", a][:, r] if is_mean else tiles["prod1", n][:]).rearrange("p u (q b) i -> p u q (b i)", q=2)
@@ -421,6 +445,9 @@ def tile_gaussian_nn_htanh_v_kernel(
         def four(*name):
             return [name + (n,) for n in range(T)]
 
+        def swapped(names):
+            return [names[n ^ 1] for n in range(len(names))]
+
         def loads(*keys):
             return [("load",) + key for key in keys]
 
@@ -461,66 +488,66 @@ def tile_gaussian_nn_htanh_v_kernel(
         def around(a, b):
             return means_first(a) + products_first(b)
 
-        sp += loads(("sig2", 0), ("e2", 0, 0), ("mu2", 0), ("sig2", 1), ("e2", 0, 1), ("mu2", 1), ("grad", 0, 0), ("e2", 1, 0), ("e2", 1, 1), ("z", 0))
-        sp += loads(("grad", 1, 0), ("sig2", 2), ("e2", 0, 2), ("mu2", 2), ("z", 1), ("e2", 1, 2))
-        sp += loads(("sig1", 0), ("e1", 0, 0), ("mu1", 0), ("z", 2), ("e1", 1, 0), ("sig1", 1), ("e1", 0, 1), ("mu1", 1), ("z", 3), ("grad", 0, 1), ("e1", 1, 1))
+        sp += loads(("sig2", 0), ("e2", 0, 0), ("mu2", 0), ("e2", 1, 0), ("sig2", 1), ("e2", 0, 1), ("mu2", 1), ("e2", 1, 1), ("grad", 0, 0), ("z", 0))
+        sp += loads(("grad", 1, 0), ("mu2", 2), ("sig2", 2), ("e2", 0, 2), ("z", 1), ("e2", 1, 2))
+        sp += loads(("sig1", 0), ("e1", 0, 0), ("z", 2), ("mu1", 0), ("e1", 1, 0), ("sig1", 1), ("e1", 0, 1), ("mu1", 1), ("z", 3), ("grad", 0, 1), ("e1", 1, 1))
         sp += loads(("sig1", 2), ("e1", 0, 2), ("z", 4), ("mu1", 2), ("grad", 1, 1), ("x", 0, 0), ("z", 5), ("x", 1, 0), ("mu1", 3), ("e1", 1, 2), ("x", 1, 1))
         sp += loads(("z", 6), ("sig1", 3), ("e1", 0, 3), ("x", 0, 1), ("e1", 1, 3))
         sp += four("store0", 0, 0) + loads(("z", 7))
-        pe += products_first(w2(0, 0, "mean2")) + means_first(w2(0, 1, "mean2")) + [("turng", 0, 0)] + around(w2(1, 0, "mean2"), w2(1, 1, "mean2"))
-        dve += [("mul2", 0, 0), ("mul2", 0, 1), ("mul2", 1, 0), ("mul2", 1, 1)] + two("emptyg", 0, 0) + quant("w2", 0, 0) + quant("g", 0, 0) + [("empty2", 1, 0, 0)]
-        act += [("sort2", 0), ("sort2", 1)] + two("empty2", 0, 0) + two("empty2", 0, 1) + two("abs", 0) + [("empty2", 1, 0, 1)] + two("empty2", 1, 1)
-        pe += four("dh", 0) + [("turng", 1, 0)] + two("turnz", 0) + four("dh", 1) + products_first(w2(0, 2, "raw2")) + means_first(w2(0, 3, "raw2"))
-        dve += four("mask", 0) + quant("w2", 1, 0) + quant("g", 1, 0) + [("mul2", 0, 2)] + dzn(0) + [("mul2", 0, 3), ("mul2", 1, 2)]
-        act += two("emptyg", 1, 0) + two("emptyz", 0) + [("abs", 1)] + two("empty2", 0, 2) + two("empty2", 0, 3)
+        pe += products_first(w2(0, 0, "mean2")) + means_first(w2(1, 0, "mean2")) + products_first(w2(0, 1, "mean2")) + [("turng", 0, 0)] + products_first(w2(1, 1, "mean2"))
+        dve += [("mul2", 0, 0), ("mul2", 1, 0), ("mul2", 0, 1), ("mul2", 1, 1)] + two("empty2", 1, 0) + two("emptyg", 0, 0) + quant("w2", 0, 0) + quant("g", 0, 0) + [("empty2", 1, 1, 0)]
+        act += [("sort2", 0), ("sort2", 1)] + two("empty2", 0, 0) + two("empty2", 0, 1) + two("abs", 0) + [("empty2", 1, 1, 1)]
+        pe += [("turng", 1, 0)] + four("dh", 0) + two("turnz", 0) + four("dh", 1) + around(w2(0, 2, "mean2"), w2(0, 3, "mean2"))
+        dve += four("mask", 0) + quant("w2", 1, 0) + quant("g", 1, 0) + [("mul2", 0, 2), ("mul2", 0, 3), ("mul2", 1, 2)] + dzn(0)
+        act += two("emptyg", 1, 0) + [("sort2", 2), ("sort2", 3)] + two("emptyz", 0) + [("abs", 1)] + two("empty2", 0, 2) + two("empty2", 0, 3)
 
-        pe += products_first(w2(1, 2, "raw2")) + two("turnz", 1) + means_first(w2(1, 3, "raw2")) + around(w1(0), w1(1))
-        dve += four("mask", 1) + [("mul1rest", 0), ("mul2", 1, 3), ("sort1", 0)] + dzn(1) + [("mul1", 1)] + quant("w2", 0, 1) + dzh(0) + [("mul1", 2), ("mul1", 3), ("sort1", 1)] + dzh(1)
-        on_pool(("mul1most", 0), ("prod1", 0), ("gin", 1, 0))
+        pe += products_first(w2(1, 2, "mean2")) + two("turnz", 1) + means_first(w2(1, 3, "mean2")) + products_first(w1(0)) + means_first(w1(1))
+        dve += swapped(four("mask", 1)) + [("mul2rest", 1, 3)] + quant("w2", 0, 1) + [("mul1", 0)] + dzn(1) + [("sort1", 0), ("mul1", 1)] + dzh(0) + [("mul1", 2), ("mul1", 3), ("sort1", 1)] + dzh(1)
+        on_pool(("mul2most", 1, 3), ("prod2", 1, 3), ("dz", 0))
         act += two("empty2", 1, 2) + [("abs", 2)] + two("emptyz", 1) + two("empty2", 1, 3) + two("empty1", 0) + two("empty1", 1)
-        pe += four("dh", 2) + around(w1(2), w1(3)) + two("turnz", 2) + open_with("mean1", 4) + [("turng", 0, 1)] + open_with("mean1", 5) + close_with("turn1", 4) + close_with("turn1", 5)
-        dve += four("mask", 2) + two("empty1", 2) + [("mul1", 5)] + quant("w2", 1, 1) + dzn(2) + [("mul1", 6), ("mul1", 7)] + dzh(2)
+        pe += four("dh", 2) + around(w1(2), w1(3)) + open_with("mean1", 4) + two("turnz", 2) + [("turng", 0, 1)] + open_with("mean1", 5) + close_with("turn1", 4) + close_with("turn1", 5)
+        dve += four("mask", 2)[::-1] + two("empty1", 2) + [("mul1", 5)] + quant("w2", 1, 1) + dzn(2) + [("mul1", 6), ("mul1", 7)] + dzh(2)
         on_pool(("mul1", 4), ("prod1", 4), ("dzin", 1))
-        act += [("abs", 3)] + two("empty1", 3) + two("emptyz", 2) + two("emptyg", 0, 1) + two("empty1", 4) + two("empty1", 5)
+        act += [("abs", 3)] + two("empty1", 3)[::-1] + two("emptyz", 2) + two("emptyg", 0, 1)[::-1] + two("empty1", 4)[::-1] + two("empty1", 5)[::-1]
 
         pe += four("dh", 3) + around(w1(6), w1(7)) + two("turnz", 3) + open_with("mean1", 8) + [("turng", 1, 1)] + close_with("turn1", 8)
-        dve += four("mask", 3) + [("mul1rest", 8), ("sort1", 2)] + dzn(3) + quant("g", 0, 1) + quant("w1", 0, 0) + two("weave", 0, 0) + quant("w1", 1, 0) + dzh(3)
+        dve += swapped(four("mask", 3)) + [("mul1rest", 8), ("sort1", 2)] + dzn(3) + quant("g", 0, 1) + quant("w1", 0, 0) + two("weave", 0, 0) + quant("w1", 1, 0) + dzh(3)
         on_pool(("mul1most", 8), ("prod1", 8), ("dzin", 2))
-        act += [("abs", 4)] + two("empty1", 6) + two("empty1", 7) + two("emptyz", 3) + two("emptyg", 1, 1)
+        act += [("abs", 4)] + two("empty1", 6)[::-1] + two("empty1", 7)[::-1] + two("emptyz", 3) + two("emptyg", 1, 1)[::-1]
         pe += four("dh", 4) + four("dx", 0, 0)[:3] + two("turnz", 4) + means_first(w1(9)) + [("dx", 0, 0, 3)]
-        dve += four("mask", 4) + [("mul1rest", 9)] + quant("xq", 0, 0) + dzn(4) + quant("g", 1, 1) + two("weave", 1, 0) + [("sort1", 3)] + quant("xq", 1, 0) + dzh(4)
+        dve += four("mask", 4)[::-1] + [("mul1rest", 9)] + quant("xq", 0, 0) + dzn(4) + quant("g", 1, 1) + two("weave", 1, 0) + quant("xq", 1, 0) + dzh(4)
         on_pool(("mul1most", 9), ("prod1", 9), ("dzin", 3))
-        act += two("empty1", 8) + [("abs", 5)] + four("emptyx", 0, 0)[:3] + two("emptyz", 4) + two("empty1", 9)
+        act += two("empty1", 8)[::-1] + [("abs", 5)] + four("emptyx", 0, 0)[:3] + two("emptyz", 4) + two("empty1", 9)[::-1]
         pe += four("dh", 5) + dws("dw", 0, 0, range(4)) + two("turnz", 5) + around(w1(10), w1(11)) + dws("dw", 0, 1, range(4))
-        dve += four("mask", 5) + dws("weigh", 0, 0, range(4)) + [("mul1rest", 11)] + dzn(5) + [("mul1", 12)] + dzh(5) + dws("weigh", 0, 1, range(4))
+        dve += swapped(four("mask", 5)) + dws("weigh", 0, 0, range(4)) + [("mul1rest", 11)] + dzn(5) + [("mul1", 12)] + dzh(5) + dws("weigh", 0, 1, range(4))
         on_pool(("mul1", 10), ("prod1", 10), ("dzin", 4))
         pool.append(("mul1most", 11))
-        act += [("emptyx", 0, 0, 3)] + two("weave", 1, 1) + two("emptyz", 5) + [("abs", 6)] + two("empty1", 10) + two("empty1", 11)
+        act += [("emptyx", 0, 0, 3), ("sort1row", 3)] + two("weave", 1, 1) + two("emptyz", 5) + [("abs", 6)] + two("empty1", 10)[::-1] + two("empty1", 11)[::-1]
 
-        pe += four("dh", 6) + around(w1(12), w1(13)) + two("turnz", 6) + dws("dw", 0, 0, range(4, 8)) + dws("dw", 0, 1, range(4, 8))
-        dve += four("mask", 6) + [("mul1rest", 14)] + quant("xq", 1, 1) + quant("xq", 0, 1) + [("mul1high", 15)] + dzn(6) + dws("weigh", 0, 0, range(4, 8)) + dws("weigh", 0, 1, range(4, 8))
-        on_pool(("mul1", 13), ("prod1", 13), ("dzin", 5))
-        pool += [("mul1most", 14)]
-        act += two("weave", 0, 1) + two("empty1", 12) + two("empty1", 13) + two("emptyz", 6) + [("abs", 7)]
+        pe += four("dh", 6) + around(w1(12), w1(14)) + two("turnz", 6) + dws("dw", 0, 0, range(4, 8)) + dws("dw", 0, 1, range(4, 8))
+        dve += swapped(four("mask", 6)) + [("flatrest", 13)] + quant("xq", 1, 1) + quant("xq", 0, 1) + [("flathigh", 15)] + dzn(6) + dws("weigh", 0, 0, range(4, 8)) + dws("weigh", 0, 1, range(4, 8))
+        on_pool(("mul1", 14), ("prod1", 14), ("dzin", 5))
+        pool += [("flatmost", 13)]
+        act += two("weave", 0, 1) + two("empty1", 12)[::-1] + two("empty1", 14)[::-1] + two("emptyz", 6) + [("abs", 7)]
         pe += four("dh", 7) + dws("dw", 1, 0, range(4)) + two("turnz", 7) + dws("dw", 1, 0, range(4, 8)) + dws("dw", 1, 1, range(1))
-        dve += four("mask", 7) + dws("weigh", 1, 0, range(4)) + dzn(7) + dzh(6) + dzh(7) + [("add1", 14), ("add1", 15)]
+        dve += swapped(four("mask", 7)) + swapped(dws("weigh", 1, 0, range(4))) + dzn(7) + dzh(6) + dzh(7) + [("addraw", 13), ("addraw", 15)]
         on_pool(("sum", 0, 0), ("total", 0, 0), ("dz", 6))
-        pool += [("sum", 0, 1), ("sum", 0, 2), ("mul1low", 15)]
+        pool += [("sum", 0, 1), ("sum", 0, 2), ("flatlow", 15)]
         act += two("emptyz", 7)
         sp += four("store1", 0)[:3]
-        ring = [("dxbank", 1, 0, 0), ("dxbank", 1, 0, 1), ("w1words", 14), ("dxbank", 1, 0, 2), ("w1words", 15), ("dxbank", 1, 0, 3)]
+        ring = [("dxbank", 1, 0, 0), ("dxbank", 1, 0, 1), ("w1words", 13), ("dxbank", 1, 0, 2), ("w1words", 15), ("dxbank", 1, 0, 3)]
         for n in range(3, len(ring)):
             inherits[ring[n]] = ring[n - 3]
-        pe += four("dx", 1, 0)[:2] + [("turn1w", 14), ("dx", 1, 0, 2), ("turn1w", 15), ("dx", 1, 0, 3)]
-        dve += dws("weigh", 1, 0, range(4, 8)) + dws("weigh", 1, 1, range(1)) + quant("w1", 0, 1) + quant("w1", 1, 1)
-        act += four("emptyx", 1, 0)[:2] + [("empty1w", 14), ("emptyx", 1, 0, 2), ("empty1w", 15), ("emptyx", 1, 0, 3)]
+        pe += four("dx", 1, 0)[:2] + [("turn1w", 13), ("dx", 1, 0, 2), ("turn1w", 15), ("dx", 1, 0, 3)]
+        dve += dws("weigh", 1, 0, range(4, 8))[::-1] + dws("weigh", 1, 1, range(1)) + quant("w1", 0, 1) + quant("w1", 1, 1)
+        act += four("emptyx", 1, 0)[:2] + [("empty1w", 13), ("emptyx", 1, 0, 2), ("empty1w", 15), ("emptyx", 1, 0, 3)]
         pe += dws("dw", 1, 1, range(1, 4))
         for n in range(T):
             pe += [("dx", 0, 1, n)] + dws("dw", 1, 1, range(8)[4 + 2 * n : 6 + 2 * n])
         pe += four("dx", 1, 1)[:3] + two("dx", 1, 1, T - 1)
         dve += dws("weigh", 1, 1, range(1, 6)) + [("sum", 1, 1), ("sum", 1, 2)] + dws("weigh", 1, 1, range(6, 8)) + [("sum", 1, 3)]
         pool += [("sum", 0, 3), ("sum", 1, 0)]
-        inherits["total", 0, 3] = ("prod1", 15)
+        inherits["total", 0, 3] = ("flat1", 15)
         act += four("emptyx", 0, 1) + four("emptyx", 1, 1)[:3] + [("emptyx", 1, 1, 3, 0)]
         dve.append(("emptyx", 1, 1, 3, 1))
         sp += four("store0", 1, 0)[:2] + [("store1", 0, 3)] + four("store0", 1, 0)[2:]

from contextlib import ExitStack
from functools import partial

import concourse.mybir as mybir
from concourse.masks import make_identity

J, N, X, H, Y = 2, 1024, 1024, 1024, 512

F32 = mybir.dt.float32
BF16 = mybir.dt.bfloat16
U32 = mybir.dt.uint32
U8 = mybir.dt.uint8
E4M3 = mybir.dt.float8_e4m3fn_x4
E5M2 = mybir.dt.float8_e5m2_x4
ALU = mybir.AluOpType
ACT = mybir.ActivationFunctionType

FLOPS = J * (2 * N * Y * H + 2 * N * H * X + 2 * N * H * X)
BYTES = 2 * (N * X + 2 * X * H + J * X * H + 2 * H * Y + J * H * Y + J * N * Y) + 4 * (J * N * H + N * X + X * H)

P = 128
T = 4
K = P * T
RUN = 8

EDGE = 1.0 + 3.0 / 256.0

UNITS = [(j, q, g) for g in range(2) for q in range(2) for j in range(J)]

SHIFT = 128
SLOTS = {"load": 13, "work": 17, "z": 3, "w1in": 2, "code": 22, "wide": 4, "bank": 8}


def tile_gaussian_nn_htanh_v_kernel(
    tc, x, mu_W1, mu_b1, mu_W2, mu_b2, sig_W1, sig_b1, sig_W2, sig_b2, e_W1, e_b1, e_W2, e_b2, z1, grad_out, out_0, out_1
):
    nc = tc.nc

    with ExitStack() as ctx:
        sbuf = ctx.enter_context(tc.tile_pool(name="sbuf", bufs=1))
        psum = ctx.enter_context(tc.psum_pool(name="psum", bufs=1))

        ident_f = sbuf.tile([P, P], F32, name="ident_f", tag="ident_f", align_bytes=64, offset=128)
        make_identity(nc, ident_f[:])
        ident_b = sbuf.tile([P, P], BF16, name="ident_b", tag="ident_b", align_bytes=64, offset=640)
        nc.vector.tensor_copy(out=ident_b[:], in_=ident_f[:])
        ctx.enter_context(tc.manual_schedule())

        tiles = {}
        specs = {}
        steps = {}

        def step(name, reads, writes, work):
            steps[name] = (reads, writes, work)

        def cols(n, width=P):
            return slice(width * n, width * n + width)

        def copy(engine, out, in_):
            if engine is nc.scalar:
                nc.scalar.copy(out=out, in_=in_)
            else:
                nc.vector.tensor_copy(out=out, in_=in_)

        def load(key, kind, shape, dtype, src):
            specs[key] = (kind, shape, dtype)
            step(("load",) + key, [], [key], lambda engine: engine.dma_start(out=tiles[key][:], in_=src))

        def quantize(key, fmt, src_key, kind="code"):
            def work(engine):
                words, scales = tiles[key]
                src = tiles[src_key][:].rearrange("p c t -> p (c t)")
                engine.quantize_mx(out=words[:].bitcast(fmt), scales=scales[:], in_=src)

            specs[key] = (kind, [P, specs[src_key][1][1]], U32)
            step(("quant",) + key, [src_key], [key], work)

        def mx(bank, lhs_key, lhs_cols, lhs_fmt, rhs_key, rhs_cols, rhs_fmt, start, stop):
            lhs, rhs = tiles[lhs_key], tiles[rhs_key]
            nc.tensor.matmul_mx(
                out=bank,
                lhsT=lhs[0][:, lhs_cols].bitcast(lhs_fmt),
                lhsT_scale=lhs[1][:, lhs_cols],
                rhs=rhs[0][:, rhs_cols].bitcast(rhs_fmt),
                rhs_scale=rhs[1][:, rhs_cols],
                start=start,
                stop=stop,
            )

        def turn_part(banks, block_of, is_mean, first):
            for b in range(2):
                for t in range(T):
                    flags = dict(start=(first and t == 0), stop=(not first and t == T - 1))
                    if is_mean:
                        nc.tensor.matmul(tiles[banks[b]][:, t, :], lhsT=block_of(b, t), rhs=ident_b[:], **flags)
                    else:
                        nc.tensor.matmul(tiles[banks[b]][:, t, :], lhsT=block_of(b, t), rhs=ident_f[:], is_transpose=True, **flags)

        def banks_for(key, count, shape):
            names = [key + (b,) for b in range(count)]
            for name in names:
                specs[name] = ("bank", shape, F32)
            return names

        def w2_load(src, name, a):
            blocks = 2 if a < 2 else 4
            load(name + (min(a, 2),), "load", [P, blocks, Y], BF16, src.rearrange("(a b m) y -> a m b y", b=blocks, m=P)[a if a < 2 else 1])

        def w2_in(name, a):
            return tiles[name + (min(a, 2),)][:, cols(max(a - 2, 0), 2), :]

        def w2_rows(a):
            q, r = divmod(a, 2)
            for name, src in (("sig2", sig_W2), ("mu2", mu_W2)):
                w2_load(src, (name,), a)
            specs["mean2", a] = ("work", [P, T, 2, P], BF16)

            def sort_mean(engine):
                src = w2_in(("mu2",), a).rearrange("p b (w i t) -> p (b w) t i", t=T, i=4)
                copy(engine, tiles["mean2", a][:].rearrange("p t b (w i) -> p (b w) t i", i=4), src)

            step(("sort2", a), [("mu2", min(a, 2))], [("mean2", a)], sort_mean)
            for j in range(J):
                w2_sample(j, a, q, r)

        def w2_sample(j, a, q, r):
            w2_load(e_W2[j], ("e2", j), a)
            specs["prod2", j, a] = ("work", [P, T, 2, P], F32)
            specs["w2in", j, q] = ("work", [P, K, T], BF16)
            banks = banks_for(("w2bank", j, a), 2, [P, T, P])

            def multiply(places, engine):
                if engine is nc.gpsimd:
                    out = tiles["prod2", j, a][:].rearrange("p t b w -> p t (b w)")[:, places]
                    noise, sig = (w2_in(name, a).rearrange("p b (w t) -> p t (b w)", t=T)[:, places] for name in (("e2", j), ("sig2",)))
                else:
                    out = tiles["prod2", j, a][:].rearrange("p t b (w i) -> p (b w) t i", i=2)[:, :, places]
                    noise, sig = (w2_in(name, a).rearrange("p b (w i t) -> p (b w) t i", t=T, i=2)[:, :, places] for name in (("e2", j), ("sig2",)))
                engine.tensor_tensor(out=out, in0=noise, in1=sig, op=ALU.mult)

            def turn(source, first, engine):
                block = w2_in(("mu2",), a).rearrange("p b (w t) -> p t b w", t=T) if source[0] == "mu2" else tiles[source]
                turn_part(banks, lambda b, t: block[:, t, b, :], source[0] != "prod2", first)

            def empty(b, engine):
                dst = tiles["w2in", j, q][:].rearrange("p (u b i) t -> p u b i t", u=T, i=RUN)
                src = tiles[banks[b]][:].rearrange("p t (b u i) -> p u b i t", u=T, i=RUN)
                copy(engine, dst[:, :, cols(2 * r + b, 4), :, :], src)

            for name, places in {"mul2": (0, T), "mul2most": (0, T - 1), "mul2rest": (T - 1, T), "mul2low": (0, 2), "mul2high": (2, T)}.items():
                step((name, j, a), [("e2", j, min(a, 2)), ("sig2", min(a, 2))], [("prod2", j, a)], partial(multiply, slice(*places)))
            for first in (False, True):
                for name, source in (("turn2", ("prod2", j, a)), ("mean2", ("mean2", a)), ("raw2", ("mu2", min(a, 2)))):
                    step((name, j, a, first), [source], banks, partial(turn, source, first))
            for b in range(2):
                step(("empty2", j, a, b), [banks[b]], [("w2in", j, q)], partial(empty, b))
            quantize(("w2", j, q), E4M3, ("w2in", j, q))

        def grad(j, g):
            load(("grad", j, g), "load", [P, T, Y], BF16, grad_out[j].rearrange("(g p t) y -> g p t y", g=2, t=T)[g])
            specs["gin", j, g] = ("work", [P, K, T], BF16)
            banks = banks_for(("gbank", j, g), 2, [P, 2, 2, P])

            def turn(engine):
                words = tiles["grad", j, g][:].rearrange("p t y -> p (t y)").bitcast(F32).rearrange("p (t w) -> p t w", t=T)
                for a in range(2):
                    for t in range(2):
                        for s in range(2):
                            engine.transpose(tiles[banks[a]][:, t, s, :], words[:, 2 * a + t, s::2], ident_f[:])

            def empty(a, engine):
                dst = tiles["gin", j, g][:].rearrange("p c t -> p (c t)").bitcast(F32)
                out = dst[:, cols(a, K)].rearrange("p (t m s) -> p t m s", t=2, s=2)
                copy(engine, out, tiles[banks[a]][:].rearrange("p t s m -> p t m s"))

            step(("turng", j, g), [("grad", j, g)], banks, turn)
            for a in range(2):
                step(("emptyg", j, g, a), [banks[a]], [("gin", j, g)], partial(empty, a))
            quantize(("g", j, g), E5M2, ("gin", j, g))

        def x_part(g, xh):
            load(("x", g, xh), "load", [P, T, K], BF16, x.rearrange("(g p t) w -> g p t w", g=2, t=T)[g][:, :, cols(xh, K)])
            specs["xin", g, xh] = ("work", [P, K, T], BF16)

            def interleave(n, engine):
                src = tiles["x", g, xh][:, :, cols(n, 2 * P)].rearrange("p t (c i r) -> p c t i r", i=2, r=2)
                copy(engine, tiles["xin", g, xh][:, cols(n, 2 * P), :].rearrange("p (r c i) t -> p c t i r", i=2, r=2), src)

            for n in range(2):
                step(("weave", g, xh, n), [("x", g, xh)], [("xin", g, xh)], partial(interleave, n))
            quantize(("xq", g, xh), E4M3, ("xin", g, xh))

        def w1_pair(a):
            for name, src in ((("sig1",), sig_W1), (("mu1",), mu_W1), (("e1", 0), e_W1[0]), (("e1", 1), e_W1[1])):
                load(name + (a,), "load", [P, 2, H], BF16, src.rearrange("(a m r) h -> a m r h", r=2, m=P)[a])
            specs["mean1", a] = ("work", [P, 2, T, 32, RUN], BF16)

            def sort_mean(engine):
                copy(engine, tiles["mean1", a][:], tiles["mu1", a][:].rearrange("p r (b u i) -> p r u b i", u=T, i=RUN))

            step(("sort1", a), [("mu1", a)], [("mean1", a)], sort_mean)

            def sort_row(engine):
                copy(engine, tiles["mean1", a][:, 0], tiles["mu1", a][:, 0, :].rearrange("p (b u i) -> p u b i", u=T, i=RUN))

            step(("sort1row", a), [("mu1", a)], [("mean1", a)], sort_row)

            def lay_sig(r, engine):
                for half in range(2):
                    engine.matmul(tiles["sigbank", a, r][:, cols(half, K)], lhsT=ident_b[:], rhs=tiles["sig1", a][:, r, cols(half, K)], start=True, stop=True)

            for r in range(2):
                specs["sigbank", a, r] = ("bank", [P, H], BF16)
                step(("laysig", a, r), [("sig1", a)], [("sigbank", a, r)], partial(lay_sig, r))
            for i in (2 * a, 2 * a + 1):
                for j in range(J):
                    w1_block(i, j)

        def w1_block(i, j):
            a, r = divmod(i, 2)
            xh, c = divmod(i, 4)
            n = 4 * a + 2 * j + r
            specs["prod1", n] = ("work", [P, T, 32, RUN], F32)
            specs["sum1", n] = ("work", [P, 2, 2 * P, 2], BF16)
            specs["w1in", j, xh] = ("w1in", [P, 2 * K, T], BF16)
            banks = banks_for(("w1bank", n), 2, [P, T, P])
            specs["w1words", n] = ("bank", [P, 2, 2, P], F32)

            def multiply(places, engine):
                sort = "p (b u i) -> p u b i"
                engine.tensor_tensor(
                    out=tiles["prod1", n][:, places],
                    in0=tiles["e1", j, a][:, r, :].rearrange(sort, u=T, i=RUN)[:, places],
                    in1=tiles["sig1", a][:, r, :].rearrange(sort, u=T, i=RUN)[:, places],
                    op=ALU.mult,
                )

            def multiply_bank(engine):
                sort = "p (b u i) -> p u b i"
                engine.tensor_tensor(
                    out=tiles["prod1", n][:],
                    in0=tiles["e1", j, a][:, r, :].rearrange(sort, u=T, i=RUN),
                    in1=tiles["sigbank", a, r][:].rearrange(sort, u=T, i=RUN),
                    op=ALU.mult,
                )

            step(("mul1p", n), [("e1", j, a), ("sigbank", a, r)], [("prod1", n)], multiply_bank)

            def turn(is_mean, first, engine):
                block = (tiles["mean1", a][:, r] if is_mean else tiles["prod1", n][:]).rearrange("p u (q b) i -> p u q (b i)", q=2)
                turn_part(banks, lambda q, u: block[:, u, q, :], is_mean, first)

            def empty(q, engine):
                copy(engine, tiles["w1in", j, xh][:, cols(T * q + c), :], tiles[banks[q]][:].rearrange("p u m -> p m u"))

            def add_mean(engine):
                pair = "p (s e) b i -> p s (b i) e"
                engine.tensor_tensor(
                    out=tiles["sum1", n][:],
                    in0=tiles["prod1", n][:].rearrange(pair, e=2),
                    in1=tiles["mean1", a][:, r].rearrange(pair, e=2),
                    op=ALU.add,
                )

            def multiply_flat(part, engine):
                engine.tensor_tensor(out=tiles["flat1", n][:, part], in0=tiles["e1", j, a][:, r, part], in1=tiles["sig1", a][:, r, part], op=ALU.mult)

            def add_raw(engine):
                pair = "p (b s e i) -> p b s i e"
                engine.tensor_tensor(
                    out=tiles["sum1", n][:].rearrange("p s (b i) e -> p b s i e", i=RUN),
                    in0=tiles["flat1", n][:].rearrange(pair, s=2, e=2, i=RUN),
                    in1=tiles["mu1", a][:, r, :].rearrange(pair, s=2, e=2, i=RUN),
                    op=ALU.add,
                )

            specs["flat1", n] = ("work", [P, H], F32)
            for name, part in {"flat": (0, 4), "flatmost": (0, 3), "flatrest": (3, 4), "flatlow": (0, 2), "flathigh": (2, 4)}.items():
                step((name, n), [("e1", j, a), ("sig1", a)], [("flat1", n)], partial(multiply_flat, slice(2 * P * part[0], 2 * P * part[1])))
            step(("addraw", n), [("flat1", n), ("mu1", a)], [("sum1", n)], add_raw)

            def turn_words(engine):
                words = tiles["sum1", n][:].rearrange("p s m e -> p (s m e)").bitcast(F32).rearrange("p (s q m) -> p q s m", s=2, q=2)
                for q in range(2):
                    for s in range(2):
                        engine.transpose(tiles["w1words", n][:, q, s, :], words[:, q, s, :], ident_f[:])

            def empty_words(engine):
                dst = tiles["w1in", j, xh][:].rearrange("p c t -> p (c t)").bitcast(F32).rearrange("p (q c m s) -> p q c m s", q=2, m=P, s=2)
                copy(engine, dst[:, :, c], tiles["w1words", n][:].rearrange("p q s m -> p q m s"))

            shares = {"mul1": (0, T), "mul1most": (0, T - 1), "mul1rest": (T - 1, T), "mul1low": (0, 2), "mul1high": (2, T)}
            for name, places in shares.items():
                step((name, n), [("e1", j, a), ("sig1", a)], [("prod1", n)], partial(multiply, slice(*places)))
            for first in (False, True):
                step(("turn1", n, first), [("prod1", n)], banks, partial(turn, False, first))
                step(("mean1", n, first), [("mean1", a)], banks, partial(turn, True, first))
            for q in range(2):
                step(("empty1", n, q), [banks[q]], [("w1in", j, xh)], partial(empty, q))
            step(("add1", n), [("prod1", n), ("mean1", a)], [("sum1", n)], add_mean)
            step(("turn1w", n), [("sum1", n)], [("w1words", n)], turn_words)
            step(("empty1w", n), [("w1words", n)], [("w1in", j, xh)], empty_words)
            quantize(("w1", j, xh), E4M3, ("w1in", j, xh), kind="wide")

        def unit(k):
            j, q, g = UNITS[k]
            load(("z", k), "z", [P, T, K], F32, z1[j].rearrange("(g p t) h -> g p t h", g=2, t=T)[g][:, :, cols(q, K)])
            for name in ("abs", "dz", "dzin"):
                specs[name, k] = ("work", [P, K, T], BF16)
            dh = banks_for(("dhbank", k), T, [P, T, P])
            turned = banks_for(("dzbank", k), 2, [P, T, P])

            def absolute(part, engine):
                dst = tiles["abs", k][:, part, :].rearrange("p (c i) t -> p c t i", i=2)
                src = tiles["z", k][:, :, part].rearrange("p t (c i) -> p c t i", i=2)
                engine.activation(out=dst, in_=src, func=ACT.Abs, scale=EDGE)

            def multiply(u, engine):
                for t in range(T):
                    mx(tiles[dh[u]][:, t, :], ("g", j, g), cols(t), E5M2, ("w2", j, q), cols(u), E4M3, True, True)

            def mask(u, engine):
                dz = tiles["dz", k][:].rearrange("p (u b i) t -> p u b i t", u=T, i=RUN)
                size = tiles["abs", k][:].rearrange("p (b u i) t -> p u b i t", u=T, i=RUN)
                bank = tiles[dh[u]][:].rearrange("p t (b i) -> p b i t", i=RUN)
                engine.scalar_tensor_tensor(out=dz[:, u], in0=size[:, u], scalar=EDGE, in1=bank, op0=ALU.is_lt, op1=ALU.mult)

            def turn(s, engine):
                words = tiles["dz", k][:].rearrange("p c t -> p (c t)").bitcast(F32).rearrange("p (u m s) -> p s u m", u=T, s=2)
                for u in range(T):
                    engine.transpose(tiles[turned[s]][:, u, :], words[:, s, u, :], ident_f[:])

            specs["dzs", k] = ("work", [P, 2, T, P], F32)

            def sort_words(engine):
                words = tiles["dz", k][:].rearrange("p c t -> p (c t)").bitcast(F32).rearrange("p (c m s) -> p c s m", m=4, s=2)
                copy(engine, tiles["dzs", k][:].rearrange("p s u (c m) -> p (u c) s m", m=4), words)

            def turn_sorted(s, engine):
                for u in range(T):
                    engine.transpose(tiles[turned[s]][:, u, :], tiles["dzs", k][:, s, u, :], ident_f[:])

            step(("sortz", k), [("dz", k)], [("dzs", k)], sort_words)
            for n in range(2):
                step(("turnzs", k, n), [("dzs", k)], [turned[n]], partial(turn_sorted, n))

            def empty(s, engine):
                src = tiles[turned[s]][:].bitcast(BF16).rearrange("p u (m e) -> p e m u", e=2)
                copy(engine, tiles["dzin", k][:, cols(s, K // 2), :].rearrange("p (e m) u -> p e m u", e=2), src)

            for n in range(2):
                step(("abs", k, n), [("z", k)], [("abs", k)], partial(absolute, cols(n, K // 2)))
                step(("turnz", k, n), [("dz", k)], [turned[n]], partial(turn, n))
                step(("emptyz", k, n), [turned[n]], [("dzin", k)], partial(empty, n))
            step(("abs", k), [("z", k)], [("abs", k)], partial(absolute, cols(0, K)))
            for u in range(T):
                step(("dh", k, u), [("g", j, g), ("w2", j, q)], [dh[u]], partial(multiply, u))
                step(("mask", k, u), [("abs", k), dh[u]], [("dz", k)], partial(mask, u))
            quantize(("dzn", j, q, g), E5M2, ("dz", k))
            quantize(("dzh", j, q, g), E5M2, ("dzin", k))

        def dx(g, xh, t, piece=0, pieces=1):
            key = (g, xh, t) + (piece,) * (pieces - 1)
            width = K // pieces
            bank, out = ("dxbank",) + key, ("out0",) + key
            specs[bank] = ("bank", [P, width], F32)
            specs[out] = ("work", [P, width], F32)
            passes = [(q, j) for q in range(2) for j in range(J)]

            def multiply(some, engine):
                for q, j in some:
                    columns = cols(pieces * q + piece, width)
                    mx(tiles[bank][:], ("dzh", j, q, g), cols(t), E5M2, ("w1", j, xh), columns, E4M3, (q, j) == passes[0], (q, j) == passes[-1])

            def empty(engine):
                copy(engine, tiles[out][:].rearrange("p (n m r) -> p n m r", m=P, r=2), tiles[bank][:].rearrange("p (n r m) -> p n m r", m=P, r=2))

            def store(engine):
                view = out_0.rearrange("(g p t) w -> g p t w", g=2, t=T)[g]
                engine.dma_start(out=view[:, t, cols(pieces * xh + piece, width)], in_=tiles[out][:])

            for name, some in (("dx", passes), ("dxopen", passes[:-1]), ("dxclose", passes[-1:])):
                step((name,) + key, [("dzh", j, q, g) for q, j in some] + [("w1", j, xh) for j in sorted(set(j for q, j in some))], [bank], partial(multiply, some))
            step(("emptyx",) + key, [bank], [out], empty)
            step(("store0",) + key, [out], [], store)

        def dw(q, i, j):
            bank = ("dwbank", q, i, j)
            part = ("part", q, i // 2, j)
            specs[bank] = ("bank", [P, K], F32)
            specs[part] = ("work", [P, 2, K], F32)
            natural = "p (b u i) -> p b u i"

            def multiply(engine):
                for g in range(2):
                    mx(tiles[bank][:], ("xq", g, i // 4), cols(i % 4), E4M3, ("dzn", j, q, g), cols(0, K), E5M2, g == 0, g == 1)

            def weigh(engine):
                engine.tensor_tensor(
                    out=tiles[part][:, i % 2, :].rearrange(natural, u=T, i=RUN),
                    in0=tiles["e1", j, i // 2][:, i % 2, cols(q, K)].rearrange(natural, u=T, i=RUN),
                    in1=tiles[bank][:].rearrange("p (u b i) -> p b u i", u=T, i=RUN),
                    op=ALU.mult,
                )

            step(("dw", q, i, j), [("xq", g, i // 4) for g in range(2)] + [("dzn", j, q, g) for g in range(2)], [bank], multiply)
            step(("weigh", q, i, j), [("e1", j, i // 2), bank], [part], weigh)

        def dw_sum(q, a):
            first, second, total = ("part", q, a, 0), ("part", q, a, 1), ("total", q, a)
            specs[total] = ("work", [P, 2, K], F32)

            def add(engine):
                engine.tensor_tensor(out=tiles[total][:], in0=tiles[first][:], in1=tiles[second][:], op=ALU.add)

            def store(engine):
                view = out_1.rearrange("(a m r) h -> a m r h", r=2, m=P)[a][:, :, cols(q, K)]
                engine.dma_start(out=view, in_=tiles[total][:])

            step(("sum", q, a), [first, second], [total], add)
            step(("store1", q, a), [total], [], store)

        for a in range(4):
            w2_rows(a)
            w1_pair(a)
            grad(*divmod(a, 2))
            x_part(*divmod(a, 2))
            for q in range(2):
                dw_sum(q, a)
        for k in range(len(UNITS)):
            unit(k)
            for half in range(2):
                dx(half, *divmod(k, T))
                for j in range(J):
                    dw(half, k, j)
        for piece in range(2):
            dx(1, 1, T - 1, piece, 2)

        pe, dve, act, pool, sp = [], [], [], [], []
        inherits = {}

        def two(*name):
            return [name + (0,), name + (1,)]

        def four(*name):
            return [name + (n,) for n in range(T)]

        def swapped(names):
            return [names[n ^ 1] for n in range(len(names))]

        def loads(*keys):
            return [("load",) + key for key in keys]

        def quant(*key):
            return [("quant",) + key]

        def dzn(k):
            return quant("dzn", *UNITS[k])

        def dzh(k):
            return quant("dzh", *UNITS[k])

        def on_pool(name, tile, after):
            pool.append(name)
            inherits[tile] = after

        def dws(kind, q, j, rows):
            return [(kind, q, i, j) for i in rows]

        def open_with(name, *key):
            return [(name,) + key + (True,)]

        def close_with(name, *key):
            return [(name,) + key + (False,)]

        def w2(j, a, mean):
            return (("turn2", j, a), (mean, j, a))

        def w1(n):
            return (("turn1", n), ("mean1", n))

        def products_first(*jobs):
            return [job[0] + (True,) for job in jobs] + [job[1] + (False,) for job in jobs]

        def means_first(*jobs):
            return [job[1] + (True,) for job in jobs] + [job[0] + (False,) for job in jobs]

        def around(a, b):
            return means_first(a) + products_first(b)

        sp += loads(("sig2", 0), ("e2", 0, 0), ("mu2", 0), ("e2", 1, 0), ("sig2", 1), ("e2", 0, 1), ("mu2", 1), ("e2", 1, 1), ("grad", 0, 0), ("z", 0))
        sp += loads(("grad", 1, 0), ("mu2", 2), ("sig2", 2), ("e2", 0, 2), ("z", 1), ("e2", 1, 2))
        sp += loads(("sig1", 0), ("e1", 0, 0), ("z", 2), ("mu1", 0), ("e1", 1, 0), ("sig1", 1), ("e1", 0, 1), ("mu1", 1), ("z", 3), ("grad", 0, 1), ("e1", 1, 1))
        sp += loads(("sig1", 2), ("e1", 0, 2), ("z", 4), ("mu1", 2), ("grad", 1, 1), ("x", 0, 0), ("z", 5), ("x", 1, 0), ("mu1", 3), ("e1", 1, 2), ("x", 1, 1))
        sp += loads(("z", 6), ("sig1", 3), ("e1", 0, 3), ("x", 0, 1), ("e1", 1, 3))
        sp += four("store0", 0, 0) + loads(("z", 7))
        pe += products_first(w2(0, 0, "mean2")) + means_first(w2(1, 0, "mean2")) + products_first(w2(0, 1, "mean2")) + [("turng", 0, 0)] + products_first(w2(1, 1, "mean2"))
        dve += [("mul2", 0, 0), ("mul2", 1, 0), ("mul2", 0, 1), ("mul2", 1, 1)] + two("empty2", 1, 0) + two("emptyg", 0, 0) + quant("w2", 0, 0) + quant("g", 0, 0) + [("empty2", 1, 1, 0)]
        act += [("sort2", 0), ("sort2", 1)] + two("empty2", 0, 0) + two("empty2", 0, 1) + two("abs", 0) + [("empty2", 1, 1, 1)]
        pe += [("turng", 1, 0)] + four("dh", 0) + two("turnz", 0) + four("dh", 1) + around(w2(0, 2, "mean2"), w2(0, 3, "mean2"))
        dve += four("mask", 0) + quant("w2", 1, 0) + quant("g", 1, 0) + [("mul2", 0, 2), ("mul2", 0, 3), ("mul2", 1, 2)] + dzn(0)
        act += two("emptyg", 1, 0) + [("sort2", 2), ("sort2", 3)] + two("emptyz", 0) + [("abs", 1)] + two("empty2", 0, 2) + two("empty2", 0, 3)

        pe += products_first(w2(1, 2, "mean2")) + two("turnz", 1) + means_first(w2(1, 3, "mean2")) + products_first(w1(0)) + means_first(w1(1))
        dve += swapped(four("mask", 1)) + [("mul2rest", 1, 3)] + quant("w2", 0, 1) + [("mul1", 0)] + dzn(1) + [("sort1", 0), ("mul1", 1)] + dzh(0) + [("mul1", 2), ("mul1", 3), ("sort1", 1)] + dzh(1)
        on_pool(("mul2most", 1, 3), ("prod2", 1, 3), ("dz", 0))
        act += two("empty2", 1, 2) + [("abs", 2)] + two("emptyz", 1) + two("empty2", 1, 3) + two("empty1", 0) + two("empty1", 1)
        pe += four("dh", 2) + around(w1(2), w1(3)) + open_with("mean1", 4) + two("turnz", 2) + [("turng", 0, 1)] + open_with("mean1", 5) + close_with("turn1", 4) + close_with("turn1", 5)
        dve += four("mask", 2)[::-1] + two("empty1", 2) + [("mul1", 5)] + quant("w2", 1, 1) + dzn(2) + [("mul1", 6), ("mul1", 7)] + dzh(2)
        on_pool(("mul1", 4), ("prod1", 4), ("dzin", 1))
        act += [("abs", 3)] + two("empty1", 3)[::-1] + two("emptyz", 2) + two("emptyg", 0, 1)[::-1] + two("empty1", 4)[::-1] + two("empty1", 5)[::-1]

        pe += four("dh", 3) + around(w1(6), w1(7)) + two("turnz", 3) + open_with("mean1", 8) + [("turng", 1, 1)] + close_with("turn1", 8)
        dve += swapped(four("mask", 3)) + [("mul1rest", 8), ("sort1", 2)] + dzn(3) + quant("g", 0, 1) + quant("w1", 0, 0) + two("weave", 0, 0) + quant("w1", 1, 0) + dzh(3)
        on_pool(("mul1most", 8), ("prod1", 8), ("dzin", 2))
        act += [("abs", 4)] + two("empty1", 6)[::-1] + two("empty1", 7)[::-1] + two("emptyz", 3) + two("emptyg", 1, 1)[::-1]
        pe += four("dh", 4) + four("dx", 0, 0)[:3] + two("turnz", 4) + means_first(w1(9)) + [("dx", 0, 0, 3)]
        dve += four("mask", 4)[::-1] + [("mul1rest", 9)] + quant("xq", 0, 0) + dzn(4) + quant("g", 1, 1) + two("weave", 1, 0) + quant("xq", 1, 0) + dzh(4)
        on_pool(("mul1most", 9), ("prod1", 9), ("dzin", 3))
        act += two("empty1", 8)[::-1] + [("abs", 5)] + four("emptyx", 0, 0)[:3] + two("emptyz", 4) + two("empty1", 9)[::-1]
        pe += four("dh", 5) + dws("dw", 0, 0, range(4)) + two("turnz", 5) + around(w1(10), w1(11)) + dws("dw", 0, 1, range(4))
        dve += swapped(four("mask", 5)) + dws("weigh", 0, 0, range(4)) + [("mul1rest", 11)] + dzn(5) + [("mul1", 12)] + dzh(5) + dws("weigh", 0, 1, range(4))
        on_pool(("mul1", 10), ("prod1", 10), ("dzin", 4))
        pool.append(("mul1most", 11))
        act += [("emptyx", 0, 0, 3), ("sort1row", 3)] + two("weave", 1, 1) + two("emptyz", 5) + [("abs", 6)] + two("empty1", 10)[::-1] + two("empty1", 11)[::-1]

        pe += four("dh", 6) + around(w1(12), w1(14)) + two("turnz", 6) + dws("dw", 0, 0, range(4, 8)) + dws("dw", 0, 1, range(4, 8))
        dve += swapped(four("mask", 6)) + [("flatrest", 13)] + quant("xq", 1, 1) + quant("xq", 0, 1) + [("flathigh", 15)] + dzn(6) + dws("weigh", 0, 0, range(4, 8)) + dws("weigh", 0, 1, range(4, 8))
        on_pool(("mul1", 14), ("prod1", 14), ("dzin", 5))
        pool += [("flatmost", 13)]
        act += two("weave", 0, 1) + two("empty1", 12)[::-1] + two("empty1", 14)[::-1] + two("emptyz", 6) + [("abs", 7)]
        pe += four("dh", 7) + dws("dw", 1, 0, range(4)) + two("turnz", 7) + dws("dw", 1, 0, range(4, 8)) + dws("dw", 1, 1, range(1))
        dve += swapped(four("mask", 7)) + swapped(dws("weigh", 1, 0, range(4))) + dzn(7) + dzh(6) + dzh(7) + [("addraw", 13), ("addraw", 15)]
        on_pool(("sum", 0, 0), ("total", 0, 0), ("dz", 6))
        pool += [("sum", 0, 1), ("sum", 0, 2), ("flatlow", 15)]
        act += two("emptyz", 7)
        sp += four("store1", 0)[:3]
        ring = [("dxbank", 1, 0, 0), ("dxbank", 1, 0, 1), ("w1words", 13), ("dxbank", 1, 0, 2), ("w1words", 15), ("dxbank", 1, 0, 3)]
        for n in range(3, len(ring)):
            inherits[ring[n]] = ring[n - 3]
        pe += four("dx", 1, 0)[:2] + [("turn1w", 13), ("dx", 1, 0, 2), ("turn1w", 15), ("dx", 1, 0, 3)]
        dve += dws("weigh", 1, 0, range(4, 8))[::-1] + dws("weigh", 1, 1, range(1)) + quant("w1", 0, 1) + quant("w1", 1, 1)
        act += four("emptyx", 1, 0)[:2] + [("empty1w", 13), ("emptyx", 1, 0, 2), ("empty1w", 15), ("emptyx", 1, 0, 3)]
        pe += dws("dw", 1, 1, range(1, 4))
        for n in range(T):
            pe += [("dx", 0, 1, n)] + dws("dw", 1, 1, range(8)[4 + 2 * n : 6 + 2 * n])
        pe += four("dx", 1, 1)[:3] + two("dx", 1, 1, T - 1)
        dve += dws("weigh", 1, 1, range(1, 6)) + [("sum", 1, 1), ("sum", 1, 2)] + dws("weigh", 1, 1, range(6, 8)) + [("sum", 1, 3)]
        pool += [("sum", 0, 3), ("sum", 1, 0)]
        inherits["total", 0, 3] = ("flat1", 15)
        act += four("emptyx", 0, 1) + four("emptyx", 1, 1)[:3] + [("emptyx", 1, 1, 3, 0)]
        dve.append(("emptyx", 1, 1, 3, 1))
        sp += four("store0", 1, 0)[:2] + [("store1", 0, 3)] + four("store0", 1, 0)[2:]
        for n in range(T):
            sp += [("store0", 0, 1, n), ("store1", 1, n)]
        sp += four("store0", 1, 1)[:3] + two("store0", 1, 1, 3)

        queues = [(nc.tensor, pe), (nc.vector, dve), (nc.scalar, act), (nc.gpsimd, pool), (nc.sync, sp)]
        writers = {}
        readers = {}
        for engine, queue in queues:
            for name in queue:
                for key in steps[name][0]:
                    readers[key] = readers.get(key, 0) + 1
                for key in steps[name][1]:
                    writers[key] = writers.get(key, 0) + 1
        heirs = {old: new for new, old in inherits.items()}
        free = {kind: list(range(count)) for kind, count in SLOTS.items()}
        slots = {}

        def fresh(name):
            return [key for key in steps[name][1] if key in specs and key not in tiles]

        def ready(name):
            kinds = [specs[key][0] for key in fresh(name) if key not in inherits]
            return (
                all(writers[key] == 0 for key in steps[name][0])
                and all(len(free[kind]) >= sum(other == kind for other in kinds) for kind in kinds)
                and all(key in slots for key in fresh(name) if key in inherits)
            )

        sizes = {"load": 4096, "work": 4096, "z": 8192, "w1in": 8192, "code": 2048 + SHIFT, "wide": 4096, "code_s": 512, "wide_s": 1024}
        begins = {}
        place = 1024
        for kind, size in sizes.items():
            begins[kind] = place + (64 if kind in ("code_s", "wide_s") else 0)
            place = place + size * SLOTS[kind.replace("_s", "")]

        def offset(kind, slot):
            return begins[kind] + sizes[kind] * slot

        def take(key):
            kind, shape, dtype = specs[key]
            if key not in inherits:
                slots[key] = (kind, free[kind].pop(0))
            tag = "%s%d" % slots[key]
            if kind == "bank":
                tiles[key] = psum.tile(shape, dtype, name=key[0], tag=tag)
            elif kind in ("code", "wide"):
                at = offset(*slots[key])
                if kind == "code":
                    at = at + (SHIFT if (at % 256 == 0) == (key[0] in ("g", "dzh", "xq")) else 0)
                words = sbuf.tile(shape, U32, name=key[0], tag="%s_%d" % (kind, at), align_bytes=64, offset=at)
                scales = sbuf.tile(shape, U8, name=key[0] + "_s", tag=tag + "_s", align_bytes=64, offset=offset(kind + "_s", slots[key][1]))
                tiles[key] = (words, scales)
            else:
                tiles[key] = sbuf.tile(shape, dtype, name=key[0], tag=tag, align_bytes=256, offset=offset(*slots[key]))

        def emit(engine, name):
            reads, writes, work = steps[name]
            for key in fresh(name):
                take(key)
            work(engine)
            for key in writes:
                writers[key] -= 1
            for key in reads:
                readers[key] -= 1
                if readers[key] == 0 and key in heirs:
                    slots[heirs[key]] = slots[key]
                elif readers[key] == 0 and key in specs:
                    free[slots[key][0]].append(slots[key][1])

        while any(queue for engine, queue in queues):
            heads = [(engine, queue) for engine, queue in queues if queue and ready(queue[0])]
            assert heads, [queue[:1] for engine, queue in queues]
            for engine, queue in heads:
                if ready(queue[0]):
                    emit(engine, queue.pop(0))
